import numpy as np
import ml_dtypes


def mxq(x, axis, fmt="e4m3"):
    dtype, down = {"e4m3": (ml_dtypes.float8_e4m3fn, 7), "e5m2": (ml_dtypes.float8_e5m2, 14)}[fmt]
    v = np.moveaxis(np.asarray(x, np.float32).astype(ml_dtypes.bfloat16).astype(np.float64), axis, -1)
    blocks = v.reshape(v.shape[:-1] + (-1, 32))
    amax = np.abs(blocks).max(-1, keepdims=True)
    byte = np.maximum(np.where(amax > 0, np.frexp(amax)[1] - 1 + 127, 0) - down, 1)
    scale = np.exp2(byte - 127.0)
    codes = (blocks / scale).astype(np.float32).astype(dtype).astype(np.float64)
    return np.moveaxis((codes * scale).reshape(v.shape), -1, axis)


WIDE = False


def mx_kscale(k):
    if not WIDE:
        return np.ones(k)
    levels = np.array([10, -10, 5, -5, 0])
    a = np.random.permutation(np.resize(levels, k // 512 * 4)).reshape(k // 512, 4)
    idx = np.arange(k)
    return np.exp2(a[idx // 512, idx % 128 // 32])


BF16 = ml_dtypes.bfloat16


def bf(x):
    return np.asarray(x, np.float32).astype(BF16)


def f64(x):
    return np.asarray(x).astype(np.float64)


B, C, T, TF, CCONF, GROUPS = 48, 512, 64, 256, 512, 32
EPS = 1e-5
C2 = 2 * C


def group_norm(x, gamma, beta):
    b_, c_, t_ = x.shape
    xg = x.reshape(b_, GROUPS, c_ // GROUPS, t_)
    mu = xg.mean(axis=(2, 3), keepdims=True)
    var = xg.var(axis=(2, 3), keepdims=True)
    xg = (xg - mu) / np.sqrt(var + EPS)
    return xg.reshape(b_, c_, t_) * gamma[None, :, None] + beta[None, :, None]


def pool(fh, lo, hi):
    idx = np.arange(fh.shape[-1])
    out = np.empty((fh.shape[0], fh.shape[1], lo.shape[1]))
    for i in range(fh.shape[0]):
        mask = (idx[None, :] > lo[i][:, None] - 1.0) & (idx[None, :] <= hi[i][:, None])
        out[i] = np.where(mask[None, :, :], fh[i][:, None, :], -np.inf).max(-1)
    return np.where(np.isfinite(out), out, 0.0)


def boundary_max_pooling(feature, segments):
    tin = feature.shape[-1]
    half = feature.shape[1] // 2
    s = np.clip(segments, 0.0, tin - 1.0)
    left = pool(feature[:, :half], s[..., 0], s[..., 1])
    right = pool(feature[:, half:], s[..., 2], s[..., 3])
    return np.concatenate([left, right], axis=1)


def make_segments(n, tin):
    lo = np.random.uniform(size=(B, n, 2)) * (1.25 * tin) - 0.125 * tin
    ln = np.random.uniform(size=(B, n, 2)) * (tin / 4) + 1.0
    ln = np.where(np.random.uniform(size=(B, n, 2)) < 0.1, -ln, ln)
    hi = lo + ln
    return np.stack([lo[..., 0], hi[..., 0], lo[..., 1], hi[..., 1]], axis=-1)


def setup_inputs():
    s = mx_kscale(C)
    return {
        'feature': bf(np.random.standard_normal((B, C, T)) * s[None, :, None]),
        'segments': bf(make_segments(T, T)),
        'w_lr': bf(np.random.standard_normal((C2, C)) * C ** -0.5 / s[None, :]),
        'b_lr': bf(np.random.standard_normal(C2) * 0.3),
        'g_lr': bf(1.0 + 0.2 * np.random.standard_normal(C2)),
        'be_lr': bf(np.random.standard_normal(C2) * 0.3),
    }


def reference(feature, segments, w_lr, b_lr, g_lr, be_lr):
    y = (mxq(f64(w_lr), 1, 'e4m3') @ mxq(f64(feature), 1, 'e4m3')) + f64(b_lr)[None, :, None]
    feat2 = np.maximum(group_norm(y, f64(g_lr), f64(be_lr)), 0.0)
    return feat2, boundary_max_pooling(feat2, f64(segments))

@@ -1,0 +1,290 @@
+from contextlib import ExitStack
+
+import concourse.bass as bass
+import concourse.mybir as mybir
+from concourse.masks import make_identity
+
+F32 = mybir.dt.float32
+BF16 = mybir.dt.bfloat16
+I32 = mybir.dt.int32
+U32 = mybir.dt.uint32
+U8 = mybir.dt.uint8
+FP8X4 = mybir.dt.float8_e4m3fn_x4
+ALU = mybir.AluOpType
+ACT = mybir.ActivationFunctionType
+AX = mybir.AxisListType
+
+P = 128
+B, C, T, C2 = 48, 512, 64, 1024
+NM = 8
+NCH = B // 2
+LEV = 6
+EPS = 1e-5
+SLOT_B = 12
+FLOPS = 2 * B * C2 * C * T
+
+
+def tile_coarsepyramid_pa_kernel(tc, feature, segments, w_lr, b_lr, g_lr, be_lr, out_0, out_1):
+    nc = tc.nc
+    with ExitStack() as ctx:
+        const = ctx.enter_context(tc.tile_pool(name="const", bufs=1))
+        small = ctx.enter_context(tc.tile_pool(name="small", bufs=3))
+        ypsum = ctx.enter_context(tc.psum_pool(name="ypsum", bufs=2))
+        tpsum = ctx.enter_context(tc.psum_pool(name="tpsum", bufs=2))
+        opsum = ctx.enter_context(tc.psum_pool(name="opsum", bufs=1))
+        spsum = ctx.enter_context(tc.psum_pool(name="spsum", bufs=1))
+
+        ident = const.tile([P, P], F32)
+        make_identity(nc, ident[:])
+        tabs = [const.tile([P, LEV - 1, NM, P], F32, name="tab%d" % i) for i in range(2)]
+        for tab in tabs:
+            nc.gpsimd.memset(tab[:], 0.0)
+
+        grp = const.tile([P, 32], F32)
+        nc.vector.tensor_reduce(out=grp[:], in_=ident[:].rearrange("p (q r) -> p q r", r=4), axis=AX.X, op=ALU.add)
+        bd = const.tile([P, 32, 4], F32)
+        nc.vector.tensor_scalar(out=bd[:], in0=grp[:].unsqueeze(2).to_broadcast([P, 32, 4]),
+                                scalar1=1.0 / 2048.0, scalar2=None, op0=ALU.mult)
+        bd2 = bd[:].rearrange("p q r -> p (q r)")
+
+        vec_bf = [const.tile([P, NM], BF16, name="vec_bf%d" % i) for i in range(3)]
+        for i, v in enumerate((b_lr, g_lr, be_lr)):
+            nc.sync.dma_start(out=vec_bf[i][:], in_=v.rearrange("(p m) -> p m", m=NM))
+        seg_bf = const.tile([P, NCH, 4], BF16)
+        nc.sync.dma_start(out=seg_bf[:], in_=segments.rearrange("(j l) n s -> (l n) j s", l=2))
+
+        vec = const.tile([P, 3, NM], F32)
+        for i in range(3):
+            nc.vector.tensor_copy(out=vec[:, i, :], in_=vec_bf[i][:])
+        beta = vec[:, 0, :]
+        gamma = vec[:, 1, :]
+        shift0 = vec[:, 2, :]
+        beta2 = const.tile([P, NM], F32)
+        nc.vector.tensor_scalar(out=beta2[:], in0=beta, scalar1=2.0, scalar2=None, op0=ALU.mult)
+        bsq = const.tile([P, NM], F32)
+        nc.vector.tensor_tensor(out=bsq[:], in0=beta, in1=beta, op=ALU.mult)
+        cc = const.tile([P, 2], F32)
+        nc.vector.tensor_reduce(out=cc[:, 0:1], in_=beta, axis=AX.X, op=ALU.add)
+        nc.vector.tensor_reduce(out=cc[:, 1:2], in_=bsq[:], axis=AX.X, op=ALU.add)
+        cc64 = const.tile([P, 2], F32)
+        nc.vector.tensor_scalar(out=cc64[:], in0=cc[:], scalar1=64.0, scalar2=None, op0=ALU.mult)
+        cg_ps = spsum.tile([P, 2], F32, tag="st")
+        nc.tensor.matmul(out=cg_ps[:], lhsT=bd2, rhs=cc64[:], start=True, stop=True)
+        cg = const.tile([P, 2], F32)
+        nc.vector.tensor_copy(out=cg[:], in_=cg_ps[:])
+
+        NQ = NCH * 2
+        sf = const.tile([P, NCH * 4], F32)
+        nc.vector.tensor_copy(out=sf[:], in_=seg_bf[:].rearrange("p j s -> p (j s)"))
+        nc.vector.tensor_scalar(out=sf[:], in0=sf[:], scalar1=0.0, scalar2=float(T - 1), op0=ALU.max, op1=ALU.min)
+        si = const.tile([P, NCH * 4], I32)
+        nc.vector.tensor_copy(out=si[:], in_=sf[:])
+        sr = const.tile([P, NCH * 4], F32)
+        nc.vector.tensor_copy(out=sr[:], in_=si[:])
+        over = const.tile([P, NCH * 4], F32)
+        nc.vector.tensor_tensor(out=over[:], in0=sr[:], in1=sf[:], op=ALU.is_gt)
+        fl = const.tile([P, NQ, 2], F32)
+        nc.vector.tensor_tensor(out=fl[:].rearrange("p q e -> p (q e)"), in0=sr[:], in1=over[:], op=ALU.subtract)
+        lo = fl[:, :, 0]
+        hi = fl[:, :, 1]
+        ln = const.tile([P, NQ], F32)
+        nc.vector.tensor_tensor(out=ln[:], in0=hi, in1=lo, op=ALU.subtract)
+        nc.vector.tensor_scalar(out=ln[:], in0=ln[:], scalar1=1.0, scalar2=None, op0=ALU.add)
+        valid = const.tile([P, NQ], F32)
+        nc.vector.tensor_scalar(out=valid[:], in0=ln[:], scalar1=1.0, scalar2=None, op0=ALU.is_ge)
+        lev256 = const.tile([P, NQ], F32)
+        wid = const.tile([P, NQ], F32)
+        nc.vector.memset(lev256[:], 0.0)
+        nc.vector.memset(wid[:], 0.0)
+        step = const.tile([P, NQ], F32)
+        for k in range(1, LEV):
+            nc.vector.tensor_scalar(out=step[:], in0=ln[:], scalar1=float(2 ** k), scalar2=None, op0=ALU.is_ge)
+            nc.vector.scalar_tensor_tensor(out=lev256[:], in0=step[:], scalar=256.0, in1=lev256[:], op0=ALU.mult, op1=ALU.add)
+            nc.vector.scalar_tensor_tensor(out=wid[:], in0=step[:], scalar=float(2 ** (k - 1)), in1=wid[:], op0=ALU.mult, op1=ALU.add)
+        pid_i = const.tile([P, 1], I32)
+        nc.gpsimd.iota(pid_i[:], pattern=[[0, 1]], base=0, channel_multiplier=1)
+        low_i = const.tile([P, 1], I32)
+        nc.vector.tensor_single_scalar(out=low_i[:], in_=pid_i[:], scalar=15, op=ALU.bitwise_and)
+        pid = const.tile([P, 1], F32)
+        nc.vector.tensor_copy(out=pid[:], in_=pid_i[:])
+        low = const.tile([P, 1], F32)
+        nc.vector.tensor_copy(out=low[:], in_=low_i[:])
+        lbase = const.tile([P, 1], F32)
+        nc.vector.tensor_scalar(out=lbase[:], in0=pid[:], scalar1=64.0, scalar2=128.0, op0=ALU.is_ge, op1=ALU.mult)
+        zrow = const.tile([P, 1], F32)
+        nc.vector.tensor_scalar(out=zrow[:], in0=low[:], scalar1=2.0, scalar2=float(5 * 256 + 2 * 48), op0=ALU.mult, op1=ALU.add)
+        rows = const.tile([P, NQ, 2], F32)
+        nc.vector.scalar_tensor_tensor(out=rows[:, :, 0], in0=lo, scalar=2.0, in1=lev256[:], op0=ALU.mult, op1=ALU.add)
+        t2 = const.tile([P, NQ], F32)
+        nc.vector.tensor_tensor(out=t2[:], in0=hi, in1=wid[:], op=ALU.subtract)
+        nc.vector.scalar_tensor_tensor(out=rows[:, :, 1], in0=t2[:], scalar=2.0, in1=lev256[:], op0=ALU.mult, op1=ALU.add)
+        for e in range(2):
+            nc.vector.tensor_scalar(out=rows[:, :, e], in0=rows[:, :, e], scalar1=zrow[:, 0:1], scalar2=None, op0=ALU.subtract)
+            nc.vector.tensor_tensor(out=rows[:, :, e], in0=rows[:, :, e], in1=valid[:], op=ALU.mult)
+            nc.vector.tensor_scalar(out=rows[:, :, e], in0=rows[:, :, e], scalar1=zrow[:, 0:1], scalar2=lbase[:, 0:1], op0=ALU.add, op1=ALU.add)
+        rows4 = rows[:].rearrange("p (j h) e -> p j h e", h=2)
+        nc.vector.tensor_scalar(out=rows4[:, :, 1, :], in0=rows4[:, :, 1, :], scalar1=1.0, scalar2=None, op0=ALU.add)
+        idx = const.tile([P, NCH, 2, 2], I32)
+        nc.vector.tensor_copy(out=idx[:].rearrange("p j h e -> p (j h e)"), in_=rows[:].rearrange("p q e -> p (q e)"))
+
+        w_codes = const.tile([P, NM, P], U32, align_bytes=64)
+        w_scales = const.tile([P, NM, P], U8, align_bytes=64)
+        x_codes = const.tile([P, B * T], U32, align_bytes=64)
+        x_scales = const.tile([P, B * T], U8, align_bytes=64)
+        with tc.tile_pool(name="stage", bufs=2) as stage, tc.tile_pool(name="wstage", bufs=1) as wstage:
+            w_sb = wstage.tile([P, NM, C], BF16)
+            nc.sync.dma_start(out=w_sb[:], in_=w_lr.rearrange("(p m) k -> p m k", m=NM))
+            raws = []
+            for g in range(3):
+                raw = stage.tile([P, 16, 4, T], BF16, name="raw%d" % g, tag="raw", bufs=3)
+                nc.sync.dma_start(out=raw[:].rearrange("p b j t -> p b (j t)"),
+                                  in_=feature[16 * g:16 * g + 16].rearrange("b (p j) t -> p b (j t)", j=4))
+                raws.append(raw)
+            w_words = w_sb[:].bitcast(F32).rearrange("p m (q u) -> p m q u", u=2)
+            w_grp = wstage.tile([P, NM, P, 4], BF16, align_bytes=64)
+            w_grp32 = w_grp[:].bitcast(F32)
+            for mp in range(NM // 2):
+                wt = tpsum.tile([P, 4, P], F32, tag="tp")
+                for i in range(2):
+                    for u in range(2):
+                        nc.tensor.transpose(wt[:, 2 * i + u, :], w_words[:, 2 * mp + i, :, u], ident[:])
+                for i in range(2):
+                    nc.vector.tensor_copy(out=w_grp32[:, 2 * mp + i, :, :],
+                                          in_=wt[:, 2 * i:2 * i + 2, :].rearrange("p u r -> p r u"))
+            nc.vector.quantize_mx(out=w_codes[:].rearrange("p m c -> p (m c)").bitcast(FP8X4),
+                                  scales=w_scales[:].rearrange("p m c -> p (m c)"),
+                                  in_=w_grp[:].rearrange("p m c j -> p (m c j)"))
+            for g in range(3):
+                x_grp = stage.tile([P, 16, T, 4], BF16, align_bytes=64, tag="xg")
+                nc.vector.tensor_copy(out=x_grp[:], in_=raws[g][:].rearrange("p b j t -> p b t j"))
+                nc.vector.quantize_mx(out=x_codes[:, 1024 * g:1024 * g + 1024].bitcast(FP8X4),
+                                      scales=x_scales[:, 1024 * g:1024 * g + 1024],
+                                      in_=x_grp[:].rearrange("p b t j -> p (b t j)"))
+
+        fpool = ctx.enter_context(tc.tile_pool(name="fpool", bufs=3))
+        late = ctx.enter_context(tc.tile_pool(name="late", bufs=6))
+        rpool = ctx.enter_context(tc.tile_pool(name="rpool", bufs=2))
+        gpool = ctx.enter_context(tc.tile_pool(name="gpool", bufs=2))
+        opool = ctx.enter_context(tc.tile_pool(name="opool", bufs=2))
+
+        slots = [out_0, out_1]
+        slot_store = [o[0:SLOT_B].rearrange("b (x c) t -> (b x) (c t)", c=16).rearrange("(k r) w -> r k w", k=LEV)
+                      for o in slots]
+        slot_rows = [o[0:SLOT_B].rearrange("b (x c) t -> (b x) (c t)", c=8) for o in slots]
+
+        order = list(range(SLOT_B // 2, NCH)) + list(range(SLOT_B // 2))
+        pending = []
+        for pos, j in enumerate(order):
+            is_late = j < SLOT_B // 2
+            cols = slice(P * j, P * j + P)
+            tab = tabs[pos % 2]
+            ys = []
+            for hb in range(2):
+                y = ypsum.tile([P, 4, P], F32, name="y%d" % hb, tag="y%d" % hb)
+                for i in range(4):
+                    m = 4 * hb + i
+                    nc.tensor.matmul_mx(out=y[:, i, :], lhsT=w_codes[:, m, :].bitcast(FP8X4), lhsT_scale=w_scales[:, m, :],
+                                        rhs=x_codes[:, cols].bitcast(FP8X4), rhs_scale=x_scales[:, cols],
+                                        start=True, stop=True)
+                ys.append(y)
+            s1 = small.tile([P, NM, 2], F32)
+            acc = small.tile([P, 2, 2], F32)
+            junk = small.tile([P, 4, T], F32)
+            for hb in range(2):
+                nc.vector.tensor_reduce(out=s1[:, 4 * hb:4 * hb + 4, :].rearrange("p m l -> p (m l)"),
+                                        in_=ys[hb][:].rearrange("p m (l t) -> p (m l) t", l=2), axis=AX.X, op=ALU.add)
+                for l in range(2):
+                    nc.scalar.activation(out=junk[:], in_=ys[hb][:, :, T * l:T * l + T], func=ACT.Square,
+                                         accum_out=acc[:, hb, l:l + 1])
+            cross = small.tile([P, NM, 2], F32)
+            nc.vector.tensor_tensor(out=cross[:], in0=s1[:], in1=beta2[:].unsqueeze(2).to_broadcast([P, NM, 2]), op=ALU.mult)
+            rs = small.tile([P, 2, 2], F32)
+            nc.vector.tensor_reduce(out=rs[:, 0, :], in_=s1[:].rearrange("p m l -> p l m"), axis=AX.X, op=ALU.add)
+            nc.vector.tensor_reduce(out=rs[:, 1, :], in_=cross[:].rearrange("p m l -> p l m"), axis=AX.X, op=ALU.add)
+            nc.vector.tensor_tensor(out=rs[:, 1, :], in0=rs[:, 1, :], in1=acc[:, 0, :], op=ALU.add)
+            nc.vector.tensor_tensor(out=rs[:, 1, :], in0=rs[:, 1, :], in1=acc[:, 1, :], op=ALU.add)
+            st = spsum.tile([P, 2, 2], F32, tag="st")
+            nc.tensor.matmul(out=st[:].rearrange("p s l -> p (s l)"), lhsT=bd2, rhs=rs[:].rearrange("p s l -> p (s l)"),
+                             start=True, stop=True)
+            mv = small.tile([P, 2, 2], F32)
+            nc.vector.tensor_tensor(out=mv[:], in0=st[:], in1=cg[:].unsqueeze(2).to_broadcast([P, 2, 2]), op=ALU.add)
+            var = small.tile([P, 2], F32)
+            nc.vector.tensor_tensor(out=var[:], in0=mv[:, 0, :], in1=mv[:, 0, :], op=ALU.mult)
+            nc.vector.tensor_tensor(out=var[:], in0=mv[:, 1, :], in1=var[:], op=ALU.subtract)
+            nc.vector.tensor_scalar(out=var[:], in0=var[:], scalar1=EPS, scalar2=None, op0=ALU.add)
+            std = small.tile([P, 2], F32)
+            nc.scalar.activation(out=std[:], in_=var[:], func=ACT.Sqrt)
+            rstd = small.tile([P, 2], F32)
+            nc.vector.reciprocal(out=rstd[:], in_=std[:])
+            sc = small.tile([P, NM, 2], F32)
+            nc.vector.tensor_tensor(out=sc[:], in0=gamma.unsqueeze(2).to_broadcast([P, NM, 2]),
+                                    in1=rstd[:].unsqueeze(1).to_broadcast([P, NM, 2]), op=ALU.mult)
+            sh = small.tile([P, NM, 2], F32)
+            nc.vector.tensor_tensor(out=sh[:], in0=beta.unsqueeze(2).to_broadcast([P, NM, 2]),
+                                    in1=mv[:, 0, :].unsqueeze(1).to_broadcast([P, NM, 2]), op=ALU.subtract)
+            nc.vector.tensor_tensor(out=sh[:], in0=sh[:], in1=sc[:], op=ALU.mult)
+            nc.vector.tensor_tensor(out=sh[:], in0=sh[:], in1=shift0.unsqueeze(2).to_broadcast([P, NM, 2]), op=ALU.add)
+            if is_late:
+                f = late.tile([P, NM, P], F32, name="f_late", tag="f_late")
+            else:
+                f = fpool.tile([P, NM, P], F32, name="f", tag="f")
+            for m in range(NM):
+                for l in range(2):
+                    nc.scalar.activation(out=f[:, m, T * l:T * l + T], in_=ys[m // 4][:, m % 4, T * l:T * l + T],
+                                         func=ACT.Relu, bias=sh[:, m, l:l + 1], scale=sc[:, m, l:l + 1])
+            f_stores = [(out_0[2 * j + l].rearrange("(p m) t -> p m t", m=NM), f[:, :, T * l:T * l + T]) for l in range(2)]
+            if is_late:
+                pending.extend(f_stores)
+            else:
+                for dst, src in f_stores:
+                    nc.sync.dma_start(out=dst, in_=src)
+            for k in range(LEV - 1):
+                s = 2 ** k
+                n_ok = T - 2 * s + 1
+                if k == 0:
+                    prev = f[:].rearrange("p m (l t) -> p (m l) t", l=2)
+                else:
+                    prev = tab[:, k - 1, :, :].rearrange("p m (l t) -> p (m l) t", l=2)
+                nxt = tab[:, k, :, :].rearrange("p m (l t) -> p (m l) t", l=2)
+                nc.vector.tensor_tensor(out=nxt[:, :, 0:n_ok], in0=prev[:, :, 0:n_ok], in1=prev[:, :, s:s + n_ok], op=ALU.max)
+            r = rpool.tile([P, LEV, 2, NM, 64], F32)
+            for k in range(LEV):
+                for hb in range(2):
+                    tp = tpsum.tile([P, 4, P], F32, tag="tp")
+                    for i in range(4):
+                        m = 4 * hb + i
+                        src = f[:, m, :] if k == 0 else tab[:, k - 1, m, :]
+                        nc.tensor.transpose(tp[:, i, :], src, ident[:])
+                    dst = r[:, k, :, 4 * hb:4 * hb + 4, :]
+                    view = tp[:].rearrange("p m (h q) -> p h m q", h=2)
+                    if (2 * k + hb) % 2 == 0:
+                        nc.scalar.copy(out=dst, in_=view)
+                    else:
+                        nc.vector.tensor_copy(out=dst, in_=view)
+            nc.sync.dma_start(out=slot_store[pos % 2], in_=r[:].rearrange("p k h m q -> p k (h m q)"))
+            gc = gpool.tile([P, NM, 2, 64], F32)
+            for h in range(2):
+                ga = gpool.tile([P, C], F32, name="ga%d" % h, tag="ga%d" % h)
+                gb = gpool.tile([P, C], F32, name="gb%d" % h, tag="gb%d" % h)
+                nc.gpsimd.indirect_dma_start(out=ga[:], out_offset=None, in_=slot_rows[pos % 2],
+                                             in_offset=bass.IndirectOffsetOnAxis(ap=idx[:, j, h, 0:1], axis=0))
+                nc.gpsimd.indirect_dma_start(out=gb[:], out_offset=None, in_=slot_rows[pos % 2],
+                                             in_offset=bass.IndirectOffsetOnAxis(ap=idx[:, j, h, 1:2], axis=0))
+                nc.vector.tensor_tensor(out=gc[:, :, h, :], in0=ga[:].rearrange("p (m q) -> p m q", m=NM),
+                                        in1=gb[:].rearrange("p (m q) -> p m q", m=NM), op=ALU.max)
+            if is_late:
+                o = late.tile([P, 2, NM, T], F32, name="o_late", tag="o_late")
+            else:
+                o = opool.tile([P, 2, NM, T], F32, name="o", tag="o")
+            for hb in range(2):
+                op = opsum.tile([P, 4, P], F32, tag="op")
+                for i in range(4):
+                    nc.tensor.transpose(op[:, i, :], gc[:, 4 * hb + i, :, :].rearrange("p h q -> p (h q)"), ident[:])
+                nc.scalar.copy(out=o[:, :, 4 * hb:4 * hb + 4, :], in_=op[:].rearrange("p m (l n) -> p l m n", l=2))
+            o_store = (out_1[2 * j:2 * j + 2].rearrange("l (p m) n -> p l (m n)", m=NM), o[:].rearrange("p l m n -> p l (m n)"))
+            if is_late:
+                pending.append(o_store)
+            else:
+                nc.sync.dma_start(out=o_store[0], in_=o_store[1])
+        for dst, src in pending:
+            nc.sync.dma_start(out=dst, in_=src)

@@ -29,8 +29,8 @@ def tile_coarsepyramid_pa_kernel(tc, feature, segments, w_lr, b_lr, g_lr, be_lr,
     with ExitStack() as ctx:
         const = ctx.enter_context(tc.tile_pool(name="const", bufs=1))
         small = ctx.enter_context(tc.tile_pool(name="small", bufs=3))
-        ypsum = ctx.enter_context(tc.psum_pool(name="ypsum", bufs=2))
-        tpsum = ctx.enter_context(tc.psum_pool(name="tpsum", bufs=2))
+        ypsum = ctx.enter_context(tc.psum_pool(name="ypsum", bufs=1))
+        tpsum = ctx.enter_context(tc.psum_pool(name="tpsum", bufs=4))
         opsum = ctx.enter_context(tc.psum_pool(name="opsum", bufs=1))
         spsum = ctx.enter_context(tc.psum_pool(name="spsum", bufs=1))
 
@@ -174,10 +174,11 @@ def tile_coarsepyramid_pa_kernel(tc, feature, segments, w_lr, b_lr, g_lr, be_lr,
 
         order = list(range(SLOT_B // 2, NCH)) + list(range(SLOT_B // 2))
         pending = []
-        for pos, j in enumerate(order):
-            is_late = j < SLOT_B // 2
+        live = {}
+
+        def sums(pos):
+            j = order[pos]
             cols = slice(P * j, P * j + P)
-            tab = tabs[pos % 2]
             ys = []
             for hb in range(2):
                 y = ypsum.tile([P, 4, P], F32, name="y%d" % hb, tag="y%d" % hb)
@@ -206,6 +207,11 @@ def tile_coarsepyramid_pa_kernel(tc, feature, segments, w_lr, b_lr, g_lr, be_lr,
             st = spsum.tile([P, 2, 2], F32, tag="st")
             nc.tensor.matmul(out=st[:].rearrange("p s l -> p (s l)"), lhsT=bd2, rhs=rs[:].rearrange("p s l -> p (s l)"),
                              start=True, stop=True)
+            live[("y", pos)] = ys
+            live[("st", pos)] = st
+
+        def deviation(pos):
+            st = live[("st", pos)]
             mv = small.tile([P, 2, 2], F32)
             nc.vector.tensor_tensor(out=mv[:], in0=st[:], in1=cg[:].unsqueeze(2).to_broadcast([P, 2, 2]), op=ALU.add)
             var = small.tile([P, 2], F32)
@@ -214,8 +220,16 @@ def tile_coarsepyramid_pa_kernel(tc, feature, segments, w_lr, b_lr, g_lr, be_lr,
             nc.vector.tensor_scalar(out=var[:], in0=var[:], scalar1=EPS, scalar2=None, op0=ALU.add)
             std = small.tile([P, 2], F32)
             nc.scalar.activation(out=std[:], in_=var[:], func=ACT.Sqrt)
+            live[("mv", pos)] = mv
+            live[("std", pos)] = std
+
+        def normalise(pos):
+            j = order[pos]
+            is_late = j < SLOT_B // 2
+            ys = live[("y", pos)]
+            mv = live[("mv", pos)]
             rstd = small.tile([P, 2], F32)
-            nc.vector.reciprocal(out=rstd[:], in_=std[:])
+            nc.vector.reciprocal(out=rstd[:], in_=live[("std", pos)][:])
             sc = small.tile([P, NM, 2], F32)
             nc.vector.tensor_tensor(out=sc[:], in0=gamma.unsqueeze(2).to_broadcast([P, NM, 2]),
                                     in1=rstd[:].unsqueeze(1).to_broadcast([P, NM, 2]), op=ALU.mult)
@@ -237,39 +251,61 @@ def tile_coarsepyramid_pa_kernel(tc, feature, segments, w_lr, b_lr, g_lr, be_lr,
                 pending.extend(f_stores)
             else:
                 for dst, src in f_stores:
-                    nc.sync.dma_start(out=dst, in_=src)
-            for k in range(LEV - 1):
-                s = 2 ** k
-                n_ok = T - 2 * s + 1
-                if k == 0:
-                    prev = f[:].rearrange("p m (l t) -> p (m l) t", l=2)
+                    nc.scalar.dma_start(out=dst, in_=src)
+            live[("f", pos)] = f
+
+        def level_up(pos, k):
+            tab = tabs[pos % 2]
+            s = 2 ** k
+            n_ok = T - 2 * s + 1
+            if k == 0:
+                prev = live[("f", pos)][:].rearrange("p m (l t) -> p (m l) t", l=2)
+            else:
+                prev = tab[:, k - 1, :, :].rearrange("p m (l t) -> p (m l) t", l=2)
+            nxt = tab[:, k, :, :].rearrange("p m (l t) -> p (m l) t", l=2)
+            nc.vector.tensor_tensor(out=nxt[:, :, 0:n_ok], in0=prev[:, :, 0:n_ok], in1=prev[:, :, s:s + n_ok], op=ALU.max)
+
+        def rows_out(pos, k):
+            tab = tabs[pos % 2]
+            f = live[("f", pos)]
+            if k == 0:
+                live[("r", pos)] = rpool.tile([P, LEV, 2, NM, 64], F32, name="r", tag="r")
+            r = live[("r", pos)]
+            for hb in range(2):
+                tp = tpsum.tile([P, 4, P], F32, tag="tp")
+                for i in range(4):
+                    m = 4 * hb + i
+                    src = f[:, m, :] if k == 0 else tab[:, k - 1, m, :]
+                    nc.tensor.transpose(tp[:, i, :], src, ident[:])
+                dst = r[:, k, :, 4 * hb:4 * hb + 4, :]
+                view = tp[:].rearrange("p m (h q) -> p h m q", h=2)
+                if (2 * k + hb) % 3 == 2:
+                    nc.vector.tensor_copy(out=dst, in_=view)
                 else:
-                    prev = tab[:, k - 1, :, :].rearrange("p m (l t) -> p (m l) t", l=2)
-                nxt = tab[:, k, :, :].rearrange("p m (l t) -> p (m l) t", l=2)
-                nc.vector.tensor_tensor(out=nxt[:, :, 0:n_ok], in0=prev[:, :, 0:n_ok], in1=prev[:, :, s:s + n_ok], op=ALU.max)
-            r = rpool.tile([P, LEV, 2, NM, 64], F32)
-            for k in range(LEV):
-                for hb in range(2):
-                    tp = tpsum.tile([P, 4, P], F32, tag="tp")
-                    for i in range(4):
-                        m = 4 * hb + i
-                        src = f[:, m, :] if k == 0 else tab[:, k - 1, m, :]
-                        nc.tensor.transpose(tp[:, i, :], src, ident[:])
-                    dst = r[:, k, :, 4 * hb:4 * hb + 4, :]
-                    view = tp[:].rearrange("p m (h q) -> p h m q", h=2)
-                    if (2 * k + hb) % 2 == 0:
-                        nc.scalar.copy(out=dst, in_=view)
-                    else:
-                        nc.vector.tensor_copy(out=dst, in_=view)
-            nc.sync.dma_start(out=slot_store[pos % 2], in_=r[:].rearrange("p k h m q -> p k (h m q)"))
-            gc = gpool.tile([P, NM, 2, 64], F32)
+                    nc.scalar.copy(out=dst, in_=view)
+            if k % 2 == 1:
+                nc.sync.dma_start(out=slot_store[pos % 2][:, k - 1:k + 1, :],
+                                  in_=r[:, k - 1:k + 1, :, :, :].rearrange("p k h m q -> p k (h m q)"))
+
+        def gathers(pos):
+            j = order[pos]
+            got = []
             for h in range(2):
-                ga = gpool.tile([P, C], F32, name="ga%d" % h, tag="ga%d" % h)
-                gb = gpool.tile([P, C], F32, name="gb%d" % h, tag="gb%d" % h)
+                ga = gpool.tile([P, C], F32, name="ga%d" % h, tag="ga%d" % h, bufs=3)
+                gb = gpool.tile([P, C], F32, name="gb%d" % h, tag="gb%d" % h, bufs=3)
                 nc.gpsimd.indirect_dma_start(out=ga[:], out_offset=None, in_=slot_rows[pos % 2],
                                              in_offset=bass.IndirectOffsetOnAxis(ap=idx[:, j, h, 0:1], axis=0))
                 nc.gpsimd.indirect_dma_start(out=gb[:], out_offset=None, in_=slot_rows[pos % 2],
                                              in_offset=bass.IndirectOffsetOnAxis(ap=idx[:, j, h, 1:2], axis=0))
+                got.append((ga, gb))
+            live[("g", pos)] = got
+
+        def pooled(pos):
+            j = order[pos]
+            is_late = j < SLOT_B // 2
+            gc = gpool.tile([P, NM, 2, 64], F32)
+            for h in range(2):
+                ga, gb = live[("g", pos)][h]
                 nc.vector.tensor_tensor(out=gc[:, :, h, :], in0=ga[:].rearrange("p (m q) -> p m q", m=NM),
                                         in1=gb[:].rearrange("p (m q) -> p m q", m=NM), op=ALU.max)
             if is_late:
@@ -285,6 +321,32 @@ def tile_coarsepyramid_pa_kernel(tc, feature, segments, w_lr, b_lr, g_lr, be_lr,
             if is_late:
                 pending.append(o_store)
             else:
-                nc.sync.dma_start(out=o_store[0], in_=o_store[1])
-        for dst, src in pending:
-            nc.sync.dma_start(out=dst, in_=src)
+                nc.scalar.dma_start(out=o_store[0], in_=o_store[1])
+
+        with tc.manual_schedule():
+            for a in range(NCH + 3):
+                first = a < NCH
+                second = 0 <= a - 1 < NCH
+                if first:
+                    sums(a)
+                if second:
+                    rows_out(a - 1, 0)
+                    level_up(a - 1, 0)
+                    level_up(a - 1, 1)
+                if first:
+                    deviation(a)
+                if second:
+                    rows_out(a - 1, 1)
+                    level_up(a - 1, 2)
+                    level_up(a - 1, 3)
+                    level_up(a - 1, 4)
+                if first:
+                    normalise(a)
+                if second:
+                    for k in range(2, LEV):
+                        rows_out(a - 1, k)
+                    gathers(a - 1)
+                if a - 3 >= 0:
+                    pooled(a - 3)
+            for dst, src in pending:
+                nc.scalar.dma_start(out=dst, in_=src)

@@ -30,7 +30,7 @@ def tile_coarsepyramid_pa_kernel(tc, feature, segments, w_lr, b_lr, g_lr, be_lr,
         const = ctx.enter_context(tc.tile_pool(name="const", bufs=1))
         small = ctx.enter_context(tc.tile_pool(name="small", bufs=3))
         ypsum = ctx.enter_context(tc.psum_pool(name="ypsum", bufs=1))
-        tpsum = ctx.enter_context(tc.psum_pool(name="tpsum", bufs=4))
+        tpsum = ctx.enter_context(tc.psum_pool(name="tpsum", bufs=3))
         opsum = ctx.enter_context(tc.psum_pool(name="opsum", bufs=1))
         spsum = ctx.enter_context(tc.psum_pool(name="spsum", bufs=1))
 
@@ -176,83 +176,123 @@ def tile_coarsepyramid_pa_kernel(tc, feature, segments, w_lr, b_lr, g_lr, be_lr,
         pending = []
         live = {}
 
-        def sums(pos):
-            j = order[pos]
-            cols = slice(P * j, P * j + P)
-            ys = []
-            for hb in range(2):
-                y = ypsum.tile([P, 4, P], F32, name="y%d" % hb, tag="y%d" % hb)
-                for i in range(4):
-                    m = 4 * hb + i
-                    nc.tensor.matmul_mx(out=y[:, i, :], lhsT=w_codes[:, m, :].bitcast(FP8X4), lhsT_scale=w_scales[:, m, :],
-                                        rhs=x_codes[:, cols].bitcast(FP8X4), rhs_scale=x_scales[:, cols],
-                                        start=True, stop=True)
-                ys.append(y)
-            s1 = small.tile([P, NM, 2], F32)
-            acc = small.tile([P, 2, 2], F32)
-            junk = small.tile([P, 4, T], F32)
-            for hb in range(2):
-                nc.vector.tensor_reduce(out=s1[:, 4 * hb:4 * hb + 4, :].rearrange("p m l -> p (m l)"),
-                                        in_=ys[hb][:].rearrange("p m (l t) -> p (m l) t", l=2), axis=AX.X, op=ALU.add)
-                for l in range(2):
-                    nc.scalar.activation(out=junk[:], in_=ys[hb][:, :, T * l:T * l + T], func=ACT.Square,
-                                         accum_out=acc[:, hb, l:l + 1])
-            cross = small.tile([P, NM, 2], F32)
-            nc.vector.tensor_tensor(out=cross[:], in0=s1[:], in1=beta2[:].unsqueeze(2).to_broadcast([P, NM, 2]), op=ALU.mult)
-            rs = small.tile([P, 2, 2], F32)
-            nc.vector.tensor_reduce(out=rs[:, 0, :], in_=s1[:].rearrange("p m l -> p l m"), axis=AX.X, op=ALU.add)
-            nc.vector.tensor_reduce(out=rs[:, 1, :], in_=cross[:].rearrange("p m l -> p l m"), axis=AX.X, op=ALU.add)
-            nc.vector.tensor_tensor(out=rs[:, 1, :], in0=rs[:, 1, :], in1=acc[:, 0, :], op=ALU.add)
-            nc.vector.tensor_tensor(out=rs[:, 1, :], in0=rs[:, 1, :], in1=acc[:, 1, :], op=ALU.add)
-            st = spsum.tile([P, 2, 2], F32, tag="st")
-            nc.tensor.matmul(out=st[:].rearrange("p s l -> p (s l)"), lhsT=bd2, rhs=rs[:].rearrange("p s l -> p (s l)"),
-                             start=True, stop=True)
-            live[("y", pos)] = ys
-            live[("st", pos)] = st
+        def mx_passes(y, pos, hb):
+            cols = slice(P * order[pos], P * order[pos] + P)
+            for i in range(4):
+                m = 4 * hb + i
+                nc.tensor.matmul_mx(out=y[:, i, :], lhsT=w_codes[:, m, :].bitcast(FP8X4), lhsT_scale=w_scales[:, m, :],
+                                    rhs=x_codes[:, cols].bitcast(FP8X4), rhs_scale=x_scales[:, cols],
+                                    start=True, stop=True)
 
-        def deviation(pos):
-            st = live[("st", pos)]
-            mv = small.tile([P, 2, 2], F32)
-            nc.vector.tensor_tensor(out=mv[:], in0=st[:], in1=cg[:].unsqueeze(2).to_broadcast([P, 2, 2]), op=ALU.add)
-            var = small.tile([P, 2], F32)
+        def sums_mx(pos, hb):
+            if pos >= NCH:
+                return
+            ysum = ypsum.tile([P, 4, P], F32, name="ysum", tag="ysum")
+            mx_passes(ysum, pos, hb)
+            live["ysum"] = ysum
+
+        def sums(pos, hb):
+            if pos >= NCH:
+                return
+            g, e = pos // 2, pos % 2
+            if e == 0 and hb == 0:
+                live[("s1", g)] = small.tile([P, 2, NM, 2], F32, name="s1", tag="s1")
+                live[("acc", g)] = small.tile([P, 2, 2, 2], F32, name="acc", tag="acc")
+            s1 = live[("s1", g)]
+            acc = live[("acc", g)]
+            ysum = live["ysum"]
+            junk = small.tile([P, 4, T], F32)
+            nc.vector.tensor_reduce(out=s1[:, e, 4 * hb:4 * hb + 4, :].rearrange("p m l -> p (m l)"),
+                                    in_=ysum[:].rearrange("p m (l t) -> p (m l) t", l=2), axis=AX.X, op=ALU.add)
+            for l in range(2):
+                nc.scalar.activation(out=junk[:], in_=ysum[:, :, T * l:T * l + T], func=ACT.Square,
+                                     accum_out=acc[:, e, hb, l:l + 1])
+
+        def chain_a(g):
+            if g >= NCH // 2:
+                return
+            s1 = live[("s1", g)]
+            acc = live[("acc", g)]
+            cross = small.tile([P, 2, NM, 2], F32)
+            nc.vector.tensor_tensor(out=cross[:], in0=s1[:],
+                                    in1=beta2[:].unsqueeze(1).unsqueeze(3).to_broadcast([P, 2, NM, 2]), op=ALU.mult)
+            rs = small.tile([P, 2, 2, 2], F32)
+            nc.vector.tensor_reduce(out=rs[:, 0, :, :], in_=s1[:].rearrange("p e m l -> p e l m"), axis=AX.X, op=ALU.add)
+            nc.vector.tensor_reduce(out=rs[:, 1, :, :], in_=cross[:].rearrange("p e m l -> p e l m"), axis=AX.X, op=ALU.add)
+            nc.vector.tensor_tensor(out=rs[:, 1, :, :], in0=rs[:, 1, :, :], in1=acc[:, :, 0, :], op=ALU.add)
+            nc.vector.tensor_tensor(out=rs[:, 1, :, :], in0=rs[:, 1, :, :], in1=acc[:, :, 1, :], op=ALU.add)
+            st = spsum.tile([P, 2, 4], F32, tag="st")
+            nc.tensor.matmul(out=st[:].rearrange("p s x -> p (s x)"), lhsT=bd2, rhs=rs[:].rearrange("p s e l -> p (s e l)"),
+                             start=True, stop=True)
+            live[("st", g)] = st
+
+        def chain_b(g):
+            if g >= NCH // 2:
+                return
+            st = live[("st", g)]
+            mv = small.tile([P, 2, 4], F32)
+            nc.vector.tensor_tensor(out=mv[:], in0=st[:], in1=cg[:].unsqueeze(2).to_broadcast([P, 2, 4]), op=ALU.add)
+            var = small.tile([P, 4], F32)
             nc.vector.tensor_tensor(out=var[:], in0=mv[:, 0, :], in1=mv[:, 0, :], op=ALU.mult)
             nc.vector.tensor_tensor(out=var[:], in0=mv[:, 1, :], in1=var[:], op=ALU.subtract)
             nc.vector.tensor_scalar(out=var[:], in0=var[:], scalar1=EPS, scalar2=None, op0=ALU.add)
-            std = small.tile([P, 2], F32)
+            std = small.tile([P, 4], F32)
             nc.scalar.activation(out=std[:], in_=var[:], func=ACT.Sqrt)
-            live[("mv", pos)] = mv
-            live[("std", pos)] = std
+            live[("mv", g)] = mv
+            live[("std", g)] = std
 
-        def normalise(pos):
-            j = order[pos]
-            is_late = j < SLOT_B // 2
-            ys = live[("y", pos)]
-            mv = live[("mv", pos)]
-            rstd = small.tile([P, 2], F32)
-            nc.vector.reciprocal(out=rstd[:], in_=live[("std", pos)][:])
-            sc = small.tile([P, NM, 2], F32)
-            nc.vector.tensor_tensor(out=sc[:], in0=gamma.unsqueeze(2).to_broadcast([P, NM, 2]),
-                                    in1=rstd[:].unsqueeze(1).to_broadcast([P, NM, 2]), op=ALU.mult)
-            sh = small.tile([P, NM, 2], F32)
-            nc.vector.tensor_tensor(out=sh[:], in0=beta.unsqueeze(2).to_broadcast([P, NM, 2]),
-                                    in1=mv[:, 0, :].unsqueeze(1).to_broadcast([P, NM, 2]), op=ALU.subtract)
+        def chain_c(g):
+            if g >= NCH // 2:
+                return
+            mv = live[("mv", g)]
+            rstd = small.tile([P, 2, 2], F32)
+            nc.vector.reciprocal(out=rstd[:].rearrange("p e l -> p (e l)"), in_=live[("std", g)][:])
+            full = [P, 2, NM, 2]
+            sc = small.tile(full, F32)
+            nc.vector.tensor_tensor(out=sc[:], in0=gamma.unsqueeze(1).unsqueeze(3).to_broadcast(full),
+                                    in1=rstd[:].unsqueeze(2).to_broadcast(full), op=ALU.mult)
+            sh = small.tile(full, F32)
+            nc.vector.tensor_tensor(out=sh[:], in0=beta.unsqueeze(1).unsqueeze(3).to_broadcast(full),
+                                    in1=mv[:, 0, :].rearrange("p (e l) -> p e l", e=2).unsqueeze(2).to_broadcast(full),
+                                    op=ALU.subtract)
             nc.vector.tensor_tensor(out=sh[:], in0=sh[:], in1=sc[:], op=ALU.mult)
-            nc.vector.tensor_tensor(out=sh[:], in0=sh[:], in1=shift0.unsqueeze(2).to_broadcast([P, NM, 2]), op=ALU.add)
-            if is_late:
-                f = late.tile([P, NM, P], F32, name="f_late", tag="f_late")
+            nc.vector.tensor_tensor(out=sh[:], in0=sh[:], in1=shift0.unsqueeze(1).unsqueeze(3).to_broadcast(full), op=ALU.add)
+            live[("sc", g)] = sc
+            live[("sh", g)] = sh
+
+        def main_mx(pos):
+            ys = []
+            for hb in range(2):
+                y = ypsum.tile([P, 4, P], F32, name="y%d" % hb, tag="y%d" % hb)
+                mx_passes(y, pos, hb)
+                ys.append(y)
+            live[("y", pos)] = ys
+            if order[pos] < SLOT_B // 2:
+                live[("f", pos)] = late.tile([P, NM, P], F32, name="f_late", tag="f_late")
             else:
-                f = fpool.tile([P, NM, P], F32, name="f", tag="f")
-            for m in range(NM):
+                live[("f", pos)] = fpool.tile([P, NM, P], F32, name="f", tag="f")
+
+        def apply_norm(pos, hb):
+            f = live[("f", pos)]
+            y = live[("y", pos)][hb]
+            sc = live[("sc", pos // 2)]
+            sh = live[("sh", pos // 2)]
+            e = pos % 2
+            for i in range(4):
+                m = 4 * hb + i
                 for l in range(2):
-                    nc.scalar.activation(out=f[:, m, T * l:T * l + T], in_=ys[m // 4][:, m % 4, T * l:T * l + T],
-                                         func=ACT.Relu, bias=sh[:, m, l:l + 1], scale=sc[:, m, l:l + 1])
-            f_stores = [(out_0[2 * j + l].rearrange("(p m) t -> p m t", m=NM), f[:, :, T * l:T * l + T]) for l in range(2)]
-            if is_late:
-                pending.extend(f_stores)
-            else:
-                for dst, src in f_stores:
-                    nc.scalar.dma_start(out=dst, in_=src)
-            live[("f", pos)] = f
+                    nc.scalar.activation(out=f[:, m, T * l:T * l + T], in_=y[:, i, T * l:T * l + T],
+                                         func=ACT.Relu, bias=sh[:, e, m, l:l + 1], scale=sc[:, e, m, l:l + 1])
+
+        def store_feat(pos):
+            j = order[pos]
+            f = live[("f", pos)]
+            for l in range(2):
+                pair = (out_0[2 * j + l].rearrange("(p m) t -> p m t", m=NM), f[:, :, T * l:T * l + T])
+                if j < SLOT_B // 2:
+                    pending.append(pair)
+                else:
+                    nc.sync.dma_start(out=pair[0], in_=pair[1])
 
         def level_up(pos, k):
             tab = tabs[pos % 2]
@@ -279,7 +319,7 @@ def tile_coarsepyramid_pa_kernel(tc, feature, segments, w_lr, b_lr, g_lr, be_lr,
                     nc.tensor.transpose(tp[:, i, :], src, ident[:])
                 dst = r[:, k, :, 4 * hb:4 * hb + 4, :]
                 view = tp[:].rearrange("p m (h q) -> p h m q", h=2)
-                if (2 * k + hb) % 3 == 2:
+                if k >= 4:
                     nc.vector.tensor_copy(out=dst, in_=view)
                 else:
                     nc.scalar.copy(out=dst, in_=view)
@@ -300,53 +340,86 @@ def tile_coarsepyramid_pa_kernel(tc, feature, segments, w_lr, b_lr, g_lr, be_lr,
                 got.append((ga, gb))
             live[("g", pos)] = got
 
-        def pooled(pos):
-            j = order[pos]
-            is_late = j < SLOT_B // 2
+        def window_max(pos):
             gc = gpool.tile([P, NM, 2, 64], F32)
             for h in range(2):
                 ga, gb = live[("g", pos)][h]
                 nc.vector.tensor_tensor(out=gc[:, :, h, :], in0=ga[:].rearrange("p (m q) -> p m q", m=NM),
                                         in1=gb[:].rearrange("p (m q) -> p m q", m=NM), op=ALU.max)
-            if is_late:
-                o = late.tile([P, 2, NM, T], F32, name="o_late", tag="o_late")
-            else:
-                o = opool.tile([P, 2, NM, T], F32, name="o", tag="o")
-            for hb in range(2):
-                op = opsum.tile([P, 4, P], F32, tag="op")
-                for i in range(4):
-                    nc.tensor.transpose(op[:, i, :], gc[:, 4 * hb + i, :, :].rearrange("p h q -> p (h q)"), ident[:])
-                nc.scalar.copy(out=o[:, :, 4 * hb:4 * hb + 4, :], in_=op[:].rearrange("p m (l n) -> p l m n", l=2))
-            o_store = (out_1[2 * j:2 * j + 2].rearrange("l (p m) n -> p l (m n)", m=NM), o[:].rearrange("p l m n -> p l (m n)"))
-            if is_late:
-                pending.append(o_store)
-            else:
-                nc.scalar.dma_start(out=o_store[0], in_=o_store[1])
+            live[("gc", pos)] = gc
+
+        def pooled_out(pos, hb):
+            j = order[pos]
+            is_late = j < SLOT_B // 2
+            gc = live[("gc", pos)]
+            if hb == 0:
+                if is_late:
+                    live[("o", pos)] = late.tile([P, 2, NM, T], F32, name="o_late", tag="o_late")
+                else:
+                    live[("o", pos)] = opool.tile([P, 2, NM, T], F32, name="o", tag="o")
+            o = live[("o", pos)]
+            op = opsum.tile([P, 4, P], F32, tag="op")
+            for i in range(4):
+                nc.tensor.transpose(op[:, i, :], gc[:, 4 * hb + i, :, :].rearrange("p h q -> p (h q)"), ident[:])
+            nc.scalar.copy(out=o[:, :, 4 * hb:4 * hb + 4, :], in_=op[:].rearrange("p m (l n) -> p l m n", l=2))
+            if hb == 1:
+                pair = (out_1[2 * j:2 * j + 2].rearrange("l (p m) n -> p l (m n)", m=NM), o[:].rearrange("p l m n -> p l (m n)"))
+                if is_late:
+                    pending.append(pair)
+                else:
+                    nc.sync.dma_start(out=pair[0], in_=pair[1])
 
         with tc.manual_schedule():
-            for a in range(NCH + 3):
+            for pos in range(3):
+                for hb in range(2):
+                    sums_mx(pos, hb)
+                    sums(pos, hb)
+                if pos == 1:
+                    chain_a(0)
+                    chain_b(0)
+                    chain_c(0)
+            for a in range(NCH + 4):
                 first = a < NCH
                 second = 0 <= a - 1 < NCH
+                third = 0 <= a - 3 < NCH
+                fourth = 0 <= a - 4 < NCH
+                g_next = (a + 1) // 2 if a % 2 == 1 else NCH
                 if first:
-                    sums(a)
+                    main_mx(a)
+                    apply_norm(a, 0)
                 if second:
                     rows_out(a - 1, 0)
                     level_up(a - 1, 0)
-                    level_up(a - 1, 1)
-                if first:
-                    deviation(a)
+                sums_mx(a + 3, 0)
                 if second:
+                    level_up(a - 1, 1)
                     rows_out(a - 1, 1)
+                chain_a(g_next)
+                if first:
+                    apply_norm(a, 1)
+                    store_feat(a)
+                if fourth:
+                    pooled_out(a - 4, 0)
+                if second:
                     level_up(a - 1, 2)
+                    rows_out(a - 1, 2)
                     level_up(a - 1, 3)
                     level_up(a - 1, 4)
-                if first:
-                    normalise(a)
+                chain_b(g_next)
+                sums(a + 3, 0)
                 if second:
-                    for k in range(2, LEV):
-                        rows_out(a - 1, k)
+                    rows_out(a - 1, 3)
+                if fourth:
+                    pooled_out(a - 4, 1)
+                if second:
+                    rows_out(a - 1, 4)
+                sums_mx(a + 3, 1)
+                chain_c(g_next)
+                if second:
+                    rows_out(a - 1, 5)
                     gathers(a - 1)
-                if a - 3 >= 0:
-                    pooled(a - 3)
+                sums(a + 3, 1)
+                if third:
+                    window_max(a - 3)
             for dst, src in pending:
-                nc.scalar.dma_start(out=dst, in_=src)
+                nc.sync.dma_start(out=dst, in_=src)

@@ -27,18 +27,74 @@ FLOPS = 2 * B * C2 * C * T
 def tile_coarsepyramid_pa_kernel(tc, feature, segments, w_lr, b_lr, g_lr, be_lr, out_0, out_1):
     nc = tc.nc
     with ExitStack() as ctx:
+        ctx.enter_context(tc.manual_schedule())
         const = ctx.enter_context(tc.tile_pool(name="const", bufs=1))
         small = ctx.enter_context(tc.tile_pool(name="small", bufs=3))
+        stage = ctx.enter_context(tc.tile_pool(name="stage", bufs=2))
         ypsum = ctx.enter_context(tc.psum_pool(name="ypsum", bufs=1))
         tpsum = ctx.enter_context(tc.psum_pool(name="tpsum", bufs=3))
         opsum = ctx.enter_context(tc.psum_pool(name="opsum", bufs=1))
-        spsum = ctx.enter_context(tc.psum_pool(name="spsum", bufs=1))
 
+        order = list(range(SLOT_B // 2, NCH)) + list(range(SLOT_B // 2))
+        live = {}
+        held = {0: [], 1: []}
+
+        pieces = [(12, 4), (16, 8), (24, 8), (32, 8), (40, 8), (0, 8), (8, 4)]
+        x_codes = const.tile([P, B * T], U32, align_bytes=64)
+        x_scales = const.tile([P, B * T], U8, align_bytes=64)
+
+        def first_use(q):
+            return order.index(pieces[q][0] // 2)
+
+        def load_piece(q):
+            b0, nb = pieces[q]
+            raw = stage.tile([P, 8, 4, T], BF16, name="raw", tag="raw", bufs=3)
+            nc.sync.dma_start(out=raw[:, 0:nb, :, :].rearrange("p b j t -> p b (j t)"),
+                              in_=feature[b0:b0 + nb].rearrange("b (p j) t -> p b (j t)", j=4))
+            live[("raw", q)] = raw
+
+        def quantise_piece(q):
+            b0, nb = pieces[q]
+            raw = live[("raw", q)]
+            x_grp = stage.tile([P, 8, T, 4], BF16, align_bytes=64, name="x_grp", tag="x_grp")
+            nc.vector.tensor_copy(out=x_grp[:, 0:nb, :, :], in_=raw[:, 0:nb, :, :].rearrange("p b j t -> p b t j"))
+            nc.vector.quantize_mx(out=x_codes[:, T * b0:T * (b0 + nb)].bitcast(FP8X4),
+                                  scales=x_scales[:, T * b0:T * (b0 + nb)],
+                                  in_=x_grp[:, 0:nb, :, :].rearrange("p b t j -> p (b t j)"))
+
+        w_codes = const.tile([P, NM, P], U32, align_bytes=64)
+        w_scales = const.tile([P, NM, P], U8, align_bytes=64)
+        vec_bf = [const.tile([P, NM], BF16, name="vec_bf%d" % i) for i in range(3)]
+        seg_bf = const.tile([P, NCH, 4], BF16)
         ident = const.tile([P, P], F32)
-        make_identity(nc, ident[:])
-        tabs = [const.tile([P, LEV - 1, NM, P], F32, name="tab%d" % i) for i in range(2)]
-        for tab in tabs:
+        tab = const.tile([P, LEV - 1, NM, P], F32)
+        pid_i = const.tile([P, 1], I32)
+        with tc.tile_pool(name="wstage", bufs=1) as wstage:
+            w_sb = wstage.tile([P, NM, C], BF16)
+            nc.sync.dma_start(out=w_sb[:], in_=w_lr.rearrange("(p m) k -> p m k", m=NM))
+            load_piece(0)
+            load_piece(1)
+            for i, v in enumerate((b_lr, g_lr, be_lr)):
+                nc.scalar.dma_start(out=vec_bf[i][:], in_=v.rearrange("(p m) -> p m", m=NM))
+            nc.scalar.dma_start(out=seg_bf[:], in_=segments.rearrange("(j l) n s -> (l n) j s", l=2))
+            make_identity(nc, ident[:])
+            nc.gpsimd.iota(pid_i[:], pattern=[[0, 1]], base=0, channel_multiplier=1)
             nc.gpsimd.memset(tab[:], 0.0)
+
+            w_words = w_sb[:].bitcast(F32).rearrange("p m (q u) -> p m q u", u=2)
+            w_grp = wstage.tile([P, NM, P, 4], BF16, align_bytes=64)
+            w_grp32 = w_grp[:].bitcast(F32)
+            for mp in range(NM // 2):
+                wt = tpsum.tile([P, 4, P], F32, tag="tp")
+                for i in range(2):
+                    for u in range(2):
+                        nc.tensor.transpose(wt[:, 2 * i + u, :], w_words[:, 2 * mp + i, :, u], ident[:])
+                nc.vector.tensor_copy(out=w_grp32[:, 2 * mp, :, :], in_=wt[:, 0:2, :].rearrange("p u r -> p r u"))
+                nc.scalar.copy(out=w_grp32[:, 2 * mp + 1, :, :], in_=wt[:, 2:4, :].rearrange("p u r -> p r u"))
+            nc.vector.quantize_mx(out=w_codes[:].rearrange("p m c -> p (m c)").bitcast(FP8X4),
+                                  scales=w_scales[:].rearrange("p m c -> p (m c)"),
+                                  in_=w_grp[:].rearrange("p m c j -> p (m c j)"))
+        quantise_piece(0)
 
         grp = const.tile([P, 32], F32)
         nc.vector.tensor_reduce(out=grp[:], in_=ident[:].rearrange("p (q r) -> p q r", r=4), axis=AX.X, op=ALU.add)
@@ -46,13 +102,6 @@ def tile_coarsepyramid_pa_kernel(tc, feature, segments, w_lr, b_lr, g_lr, be_lr,
         nc.vector.tensor_scalar(out=bd[:], in0=grp[:].unsqueeze(2).to_broadcast([P, 32, 4]),
                                 scalar1=1.0 / 2048.0, scalar2=None, op0=ALU.mult)
         bd2 = bd[:].rearrange("p q r -> p (q r)")
-
-        vec_bf = [const.tile([P, NM], BF16, name="vec_bf%d" % i) for i in range(3)]
-        for i, v in enumerate((b_lr, g_lr, be_lr)):
-            nc.sync.dma_start(out=vec_bf[i][:], in_=v.rearrange("(p m) -> p m", m=NM))
-        seg_bf = const.tile([P, NCH, 4], BF16)
-        nc.sync.dma_start(out=seg_bf[:], in_=segments.rearrange("(j l) n s -> (l n) j s", l=2))
-
         vec = const.tile([P, 3, NM], F32)
         for i in range(3):
             nc.vector.tensor_copy(out=vec[:, i, :], in_=vec_bf[i][:])
@@ -68,100 +117,67 @@ def tile_coarsepyramid_pa_kernel(tc, feature, segments, w_lr, b_lr, g_lr, be_lr,
         nc.vector.tensor_reduce(out=cc[:, 1:2], in_=bsq[:], axis=AX.X, op=ALU.add)
         cc64 = const.tile([P, 2], F32)
         nc.vector.tensor_scalar(out=cc64[:], in0=cc[:], scalar1=64.0, scalar2=None, op0=ALU.mult)
-        cg_ps = spsum.tile([P, 2], F32, tag="st")
+        cg_ps = opsum.tile([P, 2], F32, tag="op")
         nc.tensor.matmul(out=cg_ps[:], lhsT=bd2, rhs=cc64[:], start=True, stop=True)
         cg = const.tile([P, 2], F32)
         nc.vector.tensor_copy(out=cg[:], in_=cg_ps[:])
 
-        NQ = NCH * 2
-        sf = const.tile([P, NCH * 4], F32)
-        nc.vector.tensor_copy(out=sf[:], in_=seg_bf[:].rearrange("p j s -> p (j s)"))
-        nc.vector.tensor_scalar(out=sf[:], in0=sf[:], scalar1=0.0, scalar2=float(T - 1), op0=ALU.max, op1=ALU.min)
-        si = const.tile([P, NCH * 4], I32)
-        nc.vector.tensor_copy(out=si[:], in_=sf[:])
-        sr = const.tile([P, NCH * 4], F32)
-        nc.vector.tensor_copy(out=sr[:], in_=si[:])
-        over = const.tile([P, NCH * 4], F32)
-        nc.vector.tensor_tensor(out=over[:], in0=sr[:], in1=sf[:], op=ALU.is_gt)
-        fl = const.tile([P, NQ, 2], F32)
-        nc.vector.tensor_tensor(out=fl[:].rearrange("p q e -> p (q e)"), in0=sr[:], in1=over[:], op=ALU.subtract)
-        lo = fl[:, :, 0]
-        hi = fl[:, :, 1]
-        ln = const.tile([P, NQ], F32)
-        nc.vector.tensor_tensor(out=ln[:], in0=hi, in1=lo, op=ALU.subtract)
-        nc.vector.tensor_scalar(out=ln[:], in0=ln[:], scalar1=1.0, scalar2=None, op0=ALU.add)
-        valid = const.tile([P, NQ], F32)
-        nc.vector.tensor_scalar(out=valid[:], in0=ln[:], scalar1=1.0, scalar2=None, op0=ALU.is_ge)
-        lev256 = const.tile([P, NQ], F32)
-        wid = const.tile([P, NQ], F32)
-        nc.vector.memset(lev256[:], 0.0)
-        nc.vector.memset(wid[:], 0.0)
-        step = const.tile([P, NQ], F32)
-        for k in range(1, LEV):
-            nc.vector.tensor_scalar(out=step[:], in0=ln[:], scalar1=float(2 ** k), scalar2=None, op0=ALU.is_ge)
-            nc.vector.scalar_tensor_tensor(out=lev256[:], in0=step[:], scalar=256.0, in1=lev256[:], op0=ALU.mult, op1=ALU.add)
-            nc.vector.scalar_tensor_tensor(out=wid[:], in0=step[:], scalar=float(2 ** (k - 1)), in1=wid[:], op0=ALU.mult, op1=ALU.add)
-        pid_i = const.tile([P, 1], I32)
-        nc.gpsimd.iota(pid_i[:], pattern=[[0, 1]], base=0, channel_multiplier=1)
-        low_i = const.tile([P, 1], I32)
-        nc.vector.tensor_single_scalar(out=low_i[:], in_=pid_i[:], scalar=15, op=ALU.bitwise_and)
-        pid = const.tile([P, 1], F32)
-        nc.vector.tensor_copy(out=pid[:], in_=pid_i[:])
-        low = const.tile([P, 1], F32)
-        nc.vector.tensor_copy(out=low[:], in_=low_i[:])
-        lbase = const.tile([P, 1], F32)
-        nc.vector.tensor_scalar(out=lbase[:], in0=pid[:], scalar1=64.0, scalar2=128.0, op0=ALU.is_ge, op1=ALU.mult)
-        zrow = const.tile([P, 1], F32)
-        nc.vector.tensor_scalar(out=zrow[:], in0=low[:], scalar1=2.0, scalar2=float(5 * 256 + 2 * 48), op0=ALU.mult, op1=ALU.add)
-        rows = const.tile([P, NQ, 2], F32)
-        nc.vector.scalar_tensor_tensor(out=rows[:, :, 0], in0=lo, scalar=2.0, in1=lev256[:], op0=ALU.mult, op1=ALU.add)
-        t2 = const.tile([P, NQ], F32)
-        nc.vector.tensor_tensor(out=t2[:], in0=hi, in1=wid[:], op=ALU.subtract)
-        nc.vector.scalar_tensor_tensor(out=rows[:, :, 1], in0=t2[:], scalar=2.0, in1=lev256[:], op0=ALU.mult, op1=ALU.add)
-        for e in range(2):
-            nc.vector.tensor_scalar(out=rows[:, :, e], in0=rows[:, :, e], scalar1=zrow[:, 0:1], scalar2=None, op0=ALU.subtract)
-            nc.vector.tensor_tensor(out=rows[:, :, e], in0=rows[:, :, e], in1=valid[:], op=ALU.mult)
-            nc.vector.tensor_scalar(out=rows[:, :, e], in0=rows[:, :, e], scalar1=zrow[:, 0:1], scalar2=lbase[:, 0:1], op0=ALU.add, op1=ALU.add)
-        rows4 = rows[:].rearrange("p (j h) e -> p j h e", h=2)
-        nc.vector.tensor_scalar(out=rows4[:, :, 1, :], in0=rows4[:, :, 1, :], scalar1=1.0, scalar2=None, op0=ALU.add)
         idx = const.tile([P, NCH, 2, 2], I32)
-        nc.vector.tensor_copy(out=idx[:].rearrange("p j h e -> p (j h e)"), in_=rows[:].rearrange("p q e -> p (q e)"))
 
-        w_codes = const.tile([P, NM, P], U32, align_bytes=64)
-        w_scales = const.tile([P, NM, P], U8, align_bytes=64)
-        x_codes = const.tile([P, B * T], U32, align_bytes=64)
-        x_scales = const.tile([P, B * T], U8, align_bytes=64)
-        with tc.tile_pool(name="stage", bufs=2) as stage, tc.tile_pool(name="wstage", bufs=1) as wstage:
-            w_sb = wstage.tile([P, NM, C], BF16)
-            nc.sync.dma_start(out=w_sb[:], in_=w_lr.rearrange("(p m) k -> p m k", m=NM))
-            raws = []
-            for g in range(3):
-                raw = stage.tile([P, 16, 4, T], BF16, name="raw%d" % g, tag="raw", bufs=3)
-                nc.sync.dma_start(out=raw[:].rearrange("p b j t -> p b (j t)"),
-                                  in_=feature[16 * g:16 * g + 16].rearrange("b (p j) t -> p b (j t)", j=4))
-                raws.append(raw)
-            w_words = w_sb[:].bitcast(F32).rearrange("p m (q u) -> p m q u", u=2)
-            w_grp = wstage.tile([P, NM, P, 4], BF16, align_bytes=64)
-            w_grp32 = w_grp[:].bitcast(F32)
-            for mp in range(NM // 2):
-                wt = tpsum.tile([P, 4, P], F32, tag="tp")
-                for i in range(2):
-                    for u in range(2):
-                        nc.tensor.transpose(wt[:, 2 * i + u, :], w_words[:, 2 * mp + i, :, u], ident[:])
-                for i in range(2):
-                    nc.vector.tensor_copy(out=w_grp32[:, 2 * mp + i, :, :],
-                                          in_=wt[:, 2 * i:2 * i + 2, :].rearrange("p u r -> p r u"))
-            nc.vector.quantize_mx(out=w_codes[:].rearrange("p m c -> p (m c)").bitcast(FP8X4),
-                                  scales=w_scales[:].rearrange("p m c -> p (m c)"),
-                                  in_=w_grp[:].rearrange("p m c j -> p (m c j)"))
-            for g in range(3):
-                x_grp = stage.tile([P, 16, T, 4], BF16, align_bytes=64, tag="xg")
-                nc.vector.tensor_copy(out=x_grp[:], in_=raws[g][:].rearrange("p b j t -> p b t j"))
-                nc.vector.quantize_mx(out=x_codes[:, 1024 * g:1024 * g + 1024].bitcast(FP8X4),
-                                      scales=x_scales[:, 1024 * g:1024 * g + 1024],
-                                      in_=x_grp[:].rearrange("p b t j -> p (b t j)"))
+        def gather_indices():
+            NQ = NCH * 2
+            sf = const.tile([P, NCH * 4], F32)
+            nc.vector.tensor_copy(out=sf[:], in_=seg_bf[:].rearrange("p j s -> p (j s)"))
+            nc.vector.tensor_scalar(out=sf[:], in0=sf[:], scalar1=0.0, scalar2=float(T - 1), op0=ALU.max, op1=ALU.min)
+            si = const.tile([P, NCH * 4], I32)
+            nc.vector.tensor_copy(out=si[:], in_=sf[:])
+            sr = const.tile([P, NCH * 4], F32)
+            nc.vector.tensor_copy(out=sr[:], in_=si[:])
+            over = const.tile([P, NCH * 4], F32)
+            nc.vector.tensor_tensor(out=over[:], in0=sr[:], in1=sf[:], op=ALU.is_gt)
+            fl = const.tile([P, NQ, 2], F32)
+            nc.vector.tensor_tensor(out=fl[:].rearrange("p q e -> p (q e)"), in0=sr[:], in1=over[:], op=ALU.subtract)
+            lo = fl[:, :, 0]
+            hi = fl[:, :, 1]
+            ln = const.tile([P, NQ], F32)
+            nc.vector.tensor_tensor(out=ln[:], in0=hi, in1=lo, op=ALU.subtract)
+            nc.vector.tensor_scalar(out=ln[:], in0=ln[:], scalar1=1.0, scalar2=None, op0=ALU.add)
+            valid = const.tile([P, NQ], F32)
+            nc.vector.tensor_scalar(out=valid[:], in0=ln[:], scalar1=1.0, scalar2=None, op0=ALU.is_ge)
+            lev256 = const.tile([P, NQ], F32)
+            wid = const.tile([P, NQ], F32)
+            nc.vector.memset(lev256[:], 0.0)
+            nc.vector.memset(wid[:], 0.0)
+            step = const.tile([P, NQ], F32)
+            for k in range(1, LEV):
+                nc.vector.tensor_scalar(out=step[:], in0=ln[:], scalar1=float(2 ** k), scalar2=None, op0=ALU.is_ge)
+                nc.vector.scalar_tensor_tensor(out=lev256[:], in0=step[:], scalar=256.0, in1=lev256[:], op0=ALU.mult, op1=ALU.add)
+                nc.vector.scalar_tensor_tensor(out=wid[:], in0=step[:], scalar=float(2 ** (k - 1)), in1=wid[:], op0=ALU.mult, op1=ALU.add)
+            low_i = const.tile([P, 1], I32)
+            nc.vector.tensor_single_scalar(out=low_i[:], in_=pid_i[:], scalar=15, op=ALU.bitwise_and)
+            pid = const.tile([P, 1], F32)
+            nc.vector.tensor_copy(out=pid[:], in_=pid_i[:])
+            low = const.tile([P, 1], F32)
+            nc.vector.tensor_copy(out=low[:], in_=low_i[:])
+            lbase = const.tile([P, 1], F32)
+            nc.vector.tensor_scalar(out=lbase[:], in0=pid[:], scalar1=64.0, scalar2=128.0, op0=ALU.is_ge, op1=ALU.mult)
+            zrow = const.tile([P, 1], F32)
+            nc.vector.tensor_scalar(out=zrow[:], in0=low[:], scalar1=2.0, scalar2=float(5 * 256 + 2 * 48), op0=ALU.mult, op1=ALU.add)
+            rows = const.tile([P, NQ, 2], F32)
+            nc.vector.scalar_tensor_tensor(out=rows[:, :, 0], in0=lo, scalar=2.0, in1=lev256[:], op0=ALU.mult, op1=ALU.add)
+            t2 = const.tile([P, NQ], F32)
+            nc.vector.tensor_tensor(out=t2[:], in0=hi, in1=wid[:], op=ALU.subtract)
+            nc.vector.scalar_tensor_tensor(out=rows[:, :, 1], in0=t2[:], scalar=2.0, in1=lev256[:], op0=ALU.mult, op1=ALU.add)
+            for e in range(2):
+                nc.vector.tensor_scalar(out=rows[:, :, e], in0=rows[:, :, e], scalar1=zrow[:, 0:1], scalar2=None, op0=ALU.subtract)
+                nc.vector.tensor_tensor(out=rows[:, :, e], in0=rows[:, :, e], in1=valid[:], op=ALU.mult)
+                nc.vector.tensor_scalar(out=rows[:, :, e], in0=rows[:, :, e], scalar1=zrow[:, 0:1], scalar2=lbase[:, 0:1], op0=ALU.add, op1=ALU.add)
+            rows4 = rows[:].rearrange("p (j h) e -> p j h e", h=2)
+            nc.vector.tensor_scalar(out=rows4[:, :, 1, :], in0=rows4[:, :, 1, :], scalar1=1.0, scalar2=None, op0=ALU.add)
+            nc.vector.tensor_copy(out=idx[:].rearrange("p j h e -> p (j h e)"), in_=rows[:].rearrange("p q e -> p (q e)"))
 
-        fpool = ctx.enter_context(tc.tile_pool(name="fpool", bufs=3))
+
+        fpool = ctx.enter_context(tc.tile_pool(name="fpool", bufs=2))
         late = ctx.enter_context(tc.tile_pool(name="late", bufs=6))
         rpool = ctx.enter_context(tc.tile_pool(name="rpool", bufs=2))
         gpool = ctx.enter_context(tc.tile_pool(name="gpool", bufs=2))
@@ -171,10 +187,6 @@ def tile_coarsepyramid_pa_kernel(tc, feature, segments, w_lr, b_lr, g_lr, be_lr,
         slot_store = [o[0:SLOT_B].rearrange("b (x c) t -> (b x) (c t)", c=16).rearrange("(k r) w -> r k w", k=LEV)
                       for o in slots]
         slot_rows = [o[0:SLOT_B].rearrange("b (x c) t -> (b x) (c t)", c=8) for o in slots]
-
-        order = list(range(SLOT_B // 2, NCH)) + list(range(SLOT_B // 2))
-        pending = []
-        live = {}
 
         def mx_passes(y, pos, hb):
             cols = slice(P * order[pos], P * order[pos] + P)
@@ -187,9 +199,9 @@ def tile_coarsepyramid_pa_kernel(tc, feature, segments, w_lr, b_lr, g_lr, be_lr,
         def sums_mx(pos, hb):
             if pos >= NCH:
                 return
-            ysum = ypsum.tile([P, 4, P], F32, name="ysum", tag="ysum")
+            ysum = ypsum.tile([P, 4, P], F32, name="ysum%d" % hb, tag="ysum%d" % hb)
             mx_passes(ysum, pos, hb)
-            live["ysum"] = ysum
+            live[("ysum", hb)] = ysum
 
         def sums(pos, hb):
             if pos >= NCH:
@@ -200,7 +212,7 @@ def tile_coarsepyramid_pa_kernel(tc, feature, segments, w_lr, b_lr, g_lr, be_lr,
                 live[("acc", g)] = small.tile([P, 2, 2, 2], F32, name="acc", tag="acc")
             s1 = live[("s1", g)]
             acc = live[("acc", g)]
-            ysum = live["ysum"]
+            ysum = live[("ysum", hb)]
             junk = small.tile([P, 4, T], F32)
             nc.vector.tensor_reduce(out=s1[:, e, 4 * hb:4 * hb + 4, :].rearrange("p m l -> p (m l)"),
                                     in_=ysum[:].rearrange("p m (l t) -> p (m l) t", l=2), axis=AX.X, op=ALU.add)
@@ -221,7 +233,7 @@ def tile_coarsepyramid_pa_kernel(tc, feature, segments, w_lr, b_lr, g_lr, be_lr,
             nc.vector.tensor_reduce(out=rs[:, 1, :, :], in_=cross[:].rearrange("p e m l -> p e l m"), axis=AX.X, op=ALU.add)
             nc.vector.tensor_tensor(out=rs[:, 1, :, :], in0=rs[:, 1, :, :], in1=acc[:, :, 0, :], op=ALU.add)
             nc.vector.tensor_tensor(out=rs[:, 1, :, :], in0=rs[:, 1, :, :], in1=acc[:, :, 1, :], op=ALU.add)
-            st = spsum.tile([P, 2, 4], F32, tag="st")
+            st = opsum.tile([P, 2, 4], F32, tag="op")
             nc.tensor.matmul(out=st[:].rearrange("p s x -> p (s x)"), lhsT=bd2, rhs=rs[:].rearrange("p s e l -> p (s e l)"),
                              start=True, stop=True)
             live[("st", g)] = st
@@ -267,10 +279,7 @@ def tile_coarsepyramid_pa_kernel(tc, feature, segments, w_lr, b_lr, g_lr, be_lr,
                 mx_passes(y, pos, hb)
                 ys.append(y)
             live[("y", pos)] = ys
-            if order[pos] < SLOT_B // 2:
-                live[("f", pos)] = late.tile([P, NM, P], F32, name="f_late", tag="f_late")
-            else:
-                live[("f", pos)] = fpool.tile([P, NM, P], F32, name="f", tag="f")
+            live[("f", pos)] = fpool.tile([P, NM, P], F32, name="f", tag="f")
 
         def apply_norm(pos, hb):
             f = live[("f", pos)]
@@ -284,18 +293,33 @@ def tile_coarsepyramid_pa_kernel(tc, feature, segments, w_lr, b_lr, g_lr, be_lr,
                     nc.scalar.activation(out=f[:, m, T * l:T * l + T], in_=y[:, i, T * l:T * l + T],
                                          func=ACT.Relu, bias=sh[:, e, m, l:l + 1], scale=sc[:, e, m, l:l + 1])
 
+        def send(x, dst, src):
+            if held[x] is None:
+                nc.sync.dma_start(out=dst, in_=src)
+            else:
+                held[x].append((dst, src))
+
+        def give_up_slot(x):
+            for dst, src in held[x]:
+                nc.sync.dma_start(out=dst, in_=src)
+            held[x] = None
+
         def store_feat(pos):
             j = order[pos]
+            is_late = j < SLOT_B // 2
             f = live[("f", pos)]
-            for l in range(2):
-                pair = (out_0[2 * j + l].rearrange("(p m) t -> p m t", m=NM), f[:, :, T * l:T * l + T])
-                if j < SLOT_B // 2:
-                    pending.append(pair)
-                else:
-                    nc.sync.dma_start(out=pair[0], in_=pair[1])
+            if is_late:
+                f2 = late.tile([P, 2, NM, T], F32, name="f2_late", tag="f2_late")
+            else:
+                f2 = opool.tile([P, 2, NM, T], F32, name="f2", tag="f2")
+            nc.scalar.copy(out=f2[:], in_=f[:].rearrange("p m (l t) -> p l m t", l=2))
+            dst = out_0[2 * j:2 * j + 2].rearrange("l (p m) t -> p l (m t)", m=NM)
+            if is_late:
+                send(0, dst, f2[:].rearrange("p l m t -> p l (m t)"))
+            else:
+                nc.sync.dma_start(out=dst, in_=f2[:].rearrange("p l m t -> p l (m t)"))
 
         def level_up(pos, k):
-            tab = tabs[pos % 2]
             s = 2 ** k
             n_ok = T - 2 * s + 1
             if k == 0:
@@ -306,7 +330,6 @@ def tile_coarsepyramid_pa_kernel(tc, feature, segments, w_lr, b_lr, g_lr, be_lr,
             nc.vector.tensor_tensor(out=nxt[:, :, 0:n_ok], in0=prev[:, :, 0:n_ok], in1=prev[:, :, s:s + n_ok], op=ALU.max)
 
         def rows_out(pos, k):
-            tab = tabs[pos % 2]
             f = live[("f", pos)]
             if k == 0:
                 live[("r", pos)] = rpool.tile([P, LEV, 2, NM, 64], F32, name="r", tag="r")
@@ -363,63 +386,73 @@ def tile_coarsepyramid_pa_kernel(tc, feature, segments, w_lr, b_lr, g_lr, be_lr,
                 nc.tensor.transpose(op[:, i, :], gc[:, 4 * hb + i, :, :].rearrange("p h q -> p (h q)"), ident[:])
             nc.scalar.copy(out=o[:, :, 4 * hb:4 * hb + 4, :], in_=op[:].rearrange("p m (l n) -> p l m n", l=2))
             if hb == 1:
-                pair = (out_1[2 * j:2 * j + 2].rearrange("l (p m) n -> p l (m n)", m=NM), o[:].rearrange("p l m n -> p l (m n)"))
+                dst = out_1[2 * j:2 * j + 2].rearrange("l (p m) n -> p l (m n)", m=NM)
                 if is_late:
-                    pending.append(pair)
+                    send(1, dst, o[:].rearrange("p l m n -> p l (m n)"))
                 else:
-                    nc.sync.dma_start(out=pair[0], in_=pair[1])
+                    nc.sync.dma_start(out=dst, in_=o[:].rearrange("p l m n -> p l (m n)"))
 
-        with tc.manual_schedule():
-            for pos in range(3):
+        for pos in range(2):
+            for hb in range(2):
+                sums_mx(pos, hb)
+                sums(pos, hb)
+        chain_a(0)
+        chain_b(0)
+        chain_c(0)
+        for a in range(NCH + 4):
+            first = a < NCH
+            second = 0 <= a - 1 < NCH
+            third = 0 <= a - 3 < NCH
+            fourth = 0 <= a - 4 < NCH
+            g_next = (a + 1) // 2 if a % 2 == 1 else NCH
+            for q in range(2, len(pieces)):
+                if first_use(q) - 6 == a:
+                    load_piece(q)
+            if fourth:
+                pooled_out(a - 4, 0)
+            if second:
+                rows_out(a - 1, 0)
+                level_up(a - 1, 0)
+            if first:
+                main_mx(a)
+            if second:
+                level_up(a - 1, 1)
+                rows_out(a - 1, 1)
+            if a == 0:
+                apply_norm(a, 0)
+                apply_norm(a, 1)
+                store_feat(a)
+                quantise_piece(1)
                 for hb in range(2):
-                    sums_mx(pos, hb)
-                    sums(pos, hb)
-                if pos == 1:
-                    chain_a(0)
-                    chain_b(0)
-                    chain_c(0)
-            for a in range(NCH + 4):
-                first = a < NCH
-                second = 0 <= a - 1 < NCH
-                third = 0 <= a - 3 < NCH
-                fourth = 0 <= a - 4 < NCH
-                g_next = (a + 1) // 2 if a % 2 == 1 else NCH
-                if first:
-                    main_mx(a)
-                    apply_norm(a, 0)
-                if second:
-                    rows_out(a - 1, 0)
-                    level_up(a - 1, 0)
-                sums_mx(a + 3, 0)
-                if second:
-                    level_up(a - 1, 1)
-                    rows_out(a - 1, 1)
-                chain_a(g_next)
-                if first:
-                    apply_norm(a, 1)
-                    store_feat(a)
-                if fourth:
-                    pooled_out(a - 4, 0)
-                if second:
-                    level_up(a - 1, 2)
-                    rows_out(a - 1, 2)
-                    level_up(a - 1, 3)
-                    level_up(a - 1, 4)
-                chain_b(g_next)
-                sums(a + 3, 0)
-                if second:
-                    rows_out(a - 1, 3)
-                if fourth:
-                    pooled_out(a - 4, 1)
-                if second:
-                    rows_out(a - 1, 4)
-                sums_mx(a + 3, 1)
-                chain_c(g_next)
-                if second:
-                    rows_out(a - 1, 5)
-                    gathers(a - 1)
-                sums(a + 3, 1)
-                if third:
-                    window_max(a - 3)
-            for dst, src in pending:
-                nc.sync.dma_start(out=dst, in_=src)
+                    sums_mx(2, hb)
+                    sums(2, hb)
+                gather_indices()
+            sums_mx(a + 3, 0)
+            sums_mx(a + 3, 1)
+            if second:
+                level_up(a - 1, 2)
+                rows_out(a - 1, 2)
+                level_up(a - 1, 3)
+                rows_out(a - 1, 3)
+                level_up(a - 1, 4)
+                rows_out(a - 1, 4)
+                rows_out(a - 1, 5)
+                gathers(a - 1)
+            chain_a(g_next)
+            if first and a > 0:
+                apply_norm(a, 0)
+                apply_norm(a, 1)
+                store_feat(a)
+            sums(a + 3, 0)
+            chain_b(g_next)
+            if third:
+                window_max(a - 3)
+                if a - 3 >= NCH - 2:
+                    give_up_slot((a - 3) % 2)
+            if fourth:
+                pooled_out(a - 4, 1)
+            sums(a + 3, 1)
+            chain_c(g_next)
+            for q in range(2, len(pieces)):
+                if first_use(q) - 4 == a:
+                    quantise_piece(q)

@@ -20,7 +20,11 @@ NM = 8
 NCH = B // 2
 LEV = 6
 EPS = 1e-5
-SLOT_B = 12
+L_STEP = [64, 64, 64, 64, 56, 40]
+ROW0 = [0, 128, 256, 384, 512, 624]
+N_ROWS = 704
+SLOT_B = 11
+N_LATE = 6
 FLOPS = 2 * B * C2 * C * T
 
 
@@ -32,10 +36,10 @@ def tile_coarsepyramid_pa_kernel(tc, feature, segments, w_lr, b_lr, g_lr, be_lr,
         small = ctx.enter_context(tc.tile_pool(name="small", bufs=3))
         stage = ctx.enter_context(tc.tile_pool(name="stage", bufs=2))
         ypsum = ctx.enter_context(tc.psum_pool(name="ypsum", bufs=1))
-        tpsum = ctx.enter_context(tc.psum_pool(name="tpsum", bufs=3))
-        opsum = ctx.enter_context(tc.psum_pool(name="opsum", bufs=1))
+        tpsum = ctx.enter_context(tc.psum_pool(name="tpsum", bufs=4))
+        opsum = ctx.enter_context(tc.psum_pool(name="opsum", bufs=2))
 
-        order = list(range(SLOT_B // 2, NCH)) + list(range(SLOT_B // 2))
+        order = list(range(N_LATE, NCH)) + list(range(N_LATE))
         live = {}
         held = {0: [], 1: []}
 
@@ -71,11 +75,13 @@ def tile_coarsepyramid_pa_kernel(tc, feature, segments, w_lr, b_lr, g_lr, be_lr,
         pid_i = const.tile([P, 1], I32)
         with tc.tile_pool(name="wstage", bufs=1) as wstage:
             w_sb = wstage.tile([P, NM, C], BF16)
-            nc.sync.dma_start(out=w_sb[:], in_=w_lr.rearrange("(p m) k -> p m k", m=NM))
+            nc.sync.dma_start(out=w_sb[:].rearrange("p (h i) k -> p h (i k)", h=2),
+                              in_=w_lr.rearrange("(h p i) k -> p h (i k)", h=2, i=4))
             load_piece(0)
             load_piece(1)
             for i, v in enumerate((b_lr, g_lr, be_lr)):
-                nc.scalar.dma_start(out=vec_bf[i][:], in_=v.rearrange("(p m) -> p m", m=NM))
+                nc.scalar.dma_start(out=vec_bf[i][:].rearrange("p (h i) -> p h i", h=2),
+                                    in_=v.rearrange("(h p i) -> p h i", h=2, i=4))
             nc.scalar.dma_start(out=seg_bf[:], in_=segments.rearrange("(j l) n s -> (l n) j s", l=2))
             make_identity(nc, ident[:])
             nc.gpsimd.iota(pid_i[:], pattern=[[0, 1]], base=0, channel_multiplier=1)
@@ -96,36 +102,42 @@ def tile_coarsepyramid_pa_kernel(tc, feature, segments, w_lr, b_lr, g_lr, be_lr,
                                   in_=w_grp[:].rearrange("p m c j -> p (m c j)"))
         quantise_piece(0)
 
-        grp = const.tile([P, 32], F32)
-        nc.vector.tensor_reduce(out=grp[:], in_=ident[:].rearrange("p (q r) -> p q r", r=4), axis=AX.X, op=ALU.add)
-        bd = const.tile([P, 32, 4], F32)
-        nc.vector.tensor_scalar(out=bd[:], in0=grp[:].unsqueeze(2).to_broadcast([P, 32, 4]),
+        grp = const.tile([P, 16], F32)
+        nc.vector.tensor_reduce(out=grp[:], in_=ident[:].rearrange("p (q r) -> p q r", r=8), axis=AX.X, op=ALU.add)
+        bd = const.tile([P, 16, 8], F32)
+        nc.vector.tensor_scalar(out=bd[:], in0=grp[:].unsqueeze(2).to_broadcast([P, 16, 8]),
                                 scalar1=1.0 / 2048.0, scalar2=None, op0=ALU.mult)
         bd2 = bd[:].rearrange("p q r -> p (q r)")
         vec = const.tile([P, 3, NM], F32)
         for i in range(3):
             nc.vector.tensor_copy(out=vec[:, i, :], in_=vec_bf[i][:])
-        beta = vec[:, 0, :]
-        gamma = vec[:, 1, :]
-        shift0 = vec[:, 2, :]
-        beta2 = const.tile([P, NM], F32)
-        nc.vector.tensor_scalar(out=beta2[:], in0=beta, scalar1=2.0, scalar2=None, op0=ALU.mult)
+        wide = const.tile([P, 4, 2, 2, 4, 2], F32)
+        for i in range(3):
+            for e in range(2):
+                nc.vector.tensor_copy(out=wide[:, i, :, e, :, :],
+                                      in_=vec[:, i, :].rearrange("p (h i) -> p h i", h=2).unsqueeze(3).to_broadcast([P, 2, 4, 2]))
+        nc.vector.tensor_scalar(out=wide[:, 3, :, :, :, :].rearrange("p h e i l -> p (h e i l)"),
+                                in0=wide[:, 0, :, :, :, :].rearrange("p h e i l -> p (h e i l)"), scalar1=2.0, scalar2=None, op0=ALU.mult)
+        beta_w = wide[:, 0, :, :, :, :].rearrange("p h e i l -> p (h e) i l")
+        gamma_w = wide[:, 1, :, :, :, :].rearrange("p h e i l -> p (h e) i l")
+        shift_w = wide[:, 2, :, :, :, :].rearrange("p h e i l -> p (h e) i l")
+        beta2_w = wide[:, 3, :, :, :, :].rearrange("p h e i l -> p (h e) i l")
         bsq = const.tile([P, NM], F32)
-        nc.vector.tensor_tensor(out=bsq[:], in0=beta, in1=beta, op=ALU.mult)
-        cc = const.tile([P, 2], F32)
-        nc.vector.tensor_reduce(out=cc[:, 0:1], in_=beta, axis=AX.X, op=ALU.add)
-        nc.vector.tensor_reduce(out=cc[:, 1:2], in_=bsq[:], axis=AX.X, op=ALU.add)
-        cc64 = const.tile([P, 2], F32)
-        nc.vector.tensor_scalar(out=cc64[:], in0=cc[:], scalar1=64.0, scalar2=None, op0=ALU.mult)
-        cg_ps = opsum.tile([P, 2], F32, tag="op")
+        nc.vector.tensor_tensor(out=bsq[:], in0=vec[:, 0, :], in1=vec[:, 0, :], op=ALU.mult)
+        cc = const.tile([P, 2, 2], F32)
+        nc.vector.tensor_reduce(out=cc[:, 0, :], in_=vec[:, 0, :].rearrange("p (h i) -> p h i", h=2), axis=AX.X, op=ALU.add)
+        nc.vector.tensor_reduce(out=cc[:, 1, :], in_=bsq[:].rearrange("p (h i) -> p h i", h=2), axis=AX.X, op=ALU.add)
+        cc64 = const.tile([P, 4], F32)
+        nc.vector.tensor_scalar(out=cc64[:], in0=cc[:].rearrange("p s h -> p (s h)"), scalar1=64.0, scalar2=None, op0=ALU.mult)
+        cg_ps = opsum.tile([P, 4], F32, tag="op")
         nc.tensor.matmul(out=cg_ps[:], lhsT=bd2, rhs=cc64[:], start=True, stop=True)
-        cg = const.tile([P, 2], F32)
+        cg = const.tile([P, 4], F32)
         nc.vector.tensor_copy(out=cg[:], in_=cg_ps[:])
 
         idx = const.tile([P, NCH, 2, 2], I32)
 
         def gather_indices():
-            NQ = NCH * 2
+            nq = NCH * 2
             sf = const.tile([P, NCH * 4], F32)
             nc.vector.tensor_copy(out=sf[:], in_=seg_bf[:].rearrange("p j s -> p (j s)"))
             nc.vector.tensor_scalar(out=sf[:], in0=sf[:], scalar1=0.0, scalar2=float(T - 1), op0=ALU.max, op1=ALU.min)
@@ -135,106 +147,112 @@ def tile_coarsepyramid_pa_kernel(tc, feature, segments, w_lr, b_lr, g_lr, be_lr,
             nc.vector.tensor_copy(out=sr[:], in_=si[:])
             over = const.tile([P, NCH * 4], F32)
             nc.vector.tensor_tensor(out=over[:], in0=sr[:], in1=sf[:], op=ALU.is_gt)
-            fl = const.tile([P, NQ, 2], F32)
+            fl = const.tile([P, nq, 2], F32)
             nc.vector.tensor_tensor(out=fl[:].rearrange("p q e -> p (q e)"), in0=sr[:], in1=over[:], op=ALU.subtract)
             lo = fl[:, :, 0]
             hi = fl[:, :, 1]
-            ln = const.tile([P, NQ], F32)
+            ln = const.tile([P, nq], F32)
             nc.vector.tensor_tensor(out=ln[:], in0=hi, in1=lo, op=ALU.subtract)
             nc.vector.tensor_scalar(out=ln[:], in0=ln[:], scalar1=1.0, scalar2=None, op0=ALU.add)
-            valid = const.tile([P, NQ], F32)
+            valid = const.tile([P, nq], F32)
             nc.vector.tensor_scalar(out=valid[:], in0=ln[:], scalar1=1.0, scalar2=None, op0=ALU.is_ge)
-            lev256 = const.tile([P, NQ], F32)
-            wid = const.tile([P, NQ], F32)
-            nc.vector.memset(lev256[:], 0.0)
-            nc.vector.memset(wid[:], 0.0)
-            step = const.tile([P, NQ], F32)
+            lev = const.tile([P, nq], F32)
+            wid = const.tile([P, nq], F32)
+            cut = const.tile([P, nq], F32)
+            for t_ in (lev, wid, cut):
+                nc.vector.memset(t_[:], 0.0)
+            step = const.tile([P, nq], F32)
             for k in range(1, LEV):
                 nc.vector.tensor_scalar(out=step[:], in0=ln[:], scalar1=float(2 ** k), scalar2=None, op0=ALU.is_ge)
-                nc.vector.scalar_tensor_tensor(out=lev256[:], in0=step[:], scalar=256.0, in1=lev256[:], op0=ALU.mult, op1=ALU.add)
-                nc.vector.scalar_tensor_tensor(out=wid[:], in0=step[:], scalar=float(2 ** (k - 1)), in1=wid[:], op0=ALU.mult, op1=ALU.add)
+                nc.vector.scalar_tensor_tensor(out=lev[:], in0=step[:], scalar=float(2 * (ROW0[k] - ROW0[k - 1])), in1=lev[:],
+                                               op0=ALU.mult, op1=ALU.add)
+                nc.vector.scalar_tensor_tensor(out=wid[:], in0=step[:], scalar=float(2 ** (k - 1)), in1=wid[:],
+                                               op0=ALU.mult, op1=ALU.add)
+                if L_STEP[k] != L_STEP[k - 1]:
+                    nc.vector.scalar_tensor_tensor(out=cut[:], in0=step[:], scalar=float(2 * (L_STEP[k - 1] - L_STEP[k])),
+                                                   in1=cut[:], op0=ALU.mult, op1=ALU.add)
             low_i = const.tile([P, 1], I32)
-            nc.vector.tensor_single_scalar(out=low_i[:], in_=pid_i[:], scalar=15, op=ALU.bitwise_and)
+            nc.vector.tensor_single_scalar(out=low_i[:], in_=pid_i[:], scalar=3, op=ALU.bitwise_and)
             pid = const.tile([P, 1], F32)
             nc.vector.tensor_copy(out=pid[:], in_=pid_i[:])
             low = const.tile([P, 1], F32)
             nc.vector.tensor_copy(out=low[:], in_=low_i[:])
-            lbase = const.tile([P, 1], F32)
-            nc.vector.tensor_scalar(out=lbase[:], in0=pid[:], scalar1=64.0, scalar2=128.0, op0=ALU.is_ge, op1=ALU.mult)
+            l_neg = const.tile([P, 1], F32)
+            nc.vector.tensor_scalar(out=l_neg[:], in0=pid[:], scalar1=64.0, scalar2=-1.0, op0=ALU.is_ge, op1=ALU.mult)
+            z0 = const.tile([P, 1], F32)
+            nc.vector.tensor_scalar(out=z0[:], in0=low[:], scalar1=2.0, scalar2=float(2 * (ROW0[5] + 33)), op0=ALU.mult, op1=ALU.add)
             zrow = const.tile([P, 1], F32)
-            nc.vector.tensor_scalar(out=zrow[:], in0=low[:], scalar1=2.0, scalar2=float(5 * 256 + 2 * 48), op0=ALU.mult, op1=ALU.add)
-            rows = const.tile([P, NQ, 2], F32)
-            nc.vector.scalar_tensor_tensor(out=rows[:, :, 0], in0=lo, scalar=2.0, in1=lev256[:], op0=ALU.mult, op1=ALU.add)
-            t2 = const.tile([P, NQ], F32)
+            nc.vector.scalar_tensor_tensor(out=zrow[:], in0=l_neg[:], scalar=float(-2 * L_STEP[5]), in1=z0[:], op0=ALU.mult, op1=ALU.add)
+            zrel = const.tile([P, 1], F32)
+            nc.vector.scalar_tensor_tensor(out=zrel[:], in0=l_neg[:], scalar=128.0, in1=zrow[:], op0=ALU.mult, op1=ALU.add)
+            nc.vector.scalar_tensor_tensor(out=lev[:], in0=cut[:], scalar=l_neg[:, 0:1], in1=lev[:], op0=ALU.mult, op1=ALU.add)
+            rows = const.tile([P, nq, 2], F32)
+            nc.vector.scalar_tensor_tensor(out=rows[:, :, 0], in0=lo, scalar=2.0, in1=lev[:], op0=ALU.mult, op1=ALU.add)
+            t2 = const.tile([P, nq], F32)
             nc.vector.tensor_tensor(out=t2[:], in0=hi, in1=wid[:], op=ALU.subtract)
-            nc.vector.scalar_tensor_tensor(out=rows[:, :, 1], in0=t2[:], scalar=2.0, in1=lev256[:], op0=ALU.mult, op1=ALU.add)
+            nc.vector.scalar_tensor_tensor(out=rows[:, :, 1], in0=t2[:], scalar=2.0, in1=lev[:], op0=ALU.mult, op1=ALU.add)
             for e in range(2):
-                nc.vector.tensor_scalar(out=rows[:, :, e], in0=rows[:, :, e], scalar1=zrow[:, 0:1], scalar2=None, op0=ALU.subtract)
+                nc.vector.tensor_scalar(out=rows[:, :, e], in0=rows[:, :, e], scalar1=zrel[:, 0:1], scalar2=None, op0=ALU.subtract)
                 nc.vector.tensor_tensor(out=rows[:, :, e], in0=rows[:, :, e], in1=valid[:], op=ALU.mult)
-                nc.vector.tensor_scalar(out=rows[:, :, e], in0=rows[:, :, e], scalar1=zrow[:, 0:1], scalar2=lbase[:, 0:1], op0=ALU.add, op1=ALU.add)
+                nc.vector.tensor_scalar(out=rows[:, :, e], in0=rows[:, :, e], scalar1=zrow[:, 0:1], scalar2=None, op0=ALU.add)
             rows4 = rows[:].rearrange("p (j h) e -> p j h e", h=2)
             nc.vector.tensor_scalar(out=rows4[:, :, 1, :], in0=rows4[:, :, 1, :], scalar1=1.0, scalar2=None, op0=ALU.add)
             nc.vector.tensor_copy(out=idx[:].rearrange("p j h e -> p (j h e)"), in_=rows[:].rearrange("p q e -> p (q e)"))
 
-
         fpool = ctx.enter_context(tc.tile_pool(name="fpool", bufs=2))
-        late = ctx.enter_context(tc.tile_pool(name="late", bufs=6))
+        late = ctx.enter_context(tc.tile_pool(name="late", bufs=N_LATE))
         rpool = ctx.enter_context(tc.tile_pool(name="rpool", bufs=2))
-        gpool = ctx.enter_context(tc.tile_pool(name="gpool", bufs=2))
+        gpool = ctx.enter_context(tc.tile_pool(name="gpool", bufs=3))
         opool = ctx.enter_context(tc.tile_pool(name="opool", bufs=2))
 
-        slots = [out_0, out_1]
-        slot_store = [o[0:SLOT_B].rearrange("b (x c) t -> (b x) (c t)", c=16).rearrange("(k r) w -> r k w", k=LEV)
-                      for o in slots]
-        slot_rows = [o[0:SLOT_B].rearrange("b (x c) t -> (b x) (c t)", c=8) for o in slots]
+        slot_wide = [o[0:SLOT_B].rearrange("b (x c) t -> (b x) (c t)", c=16) for o in (out_0, out_1)]
+        slot_rows = [o[0:SLOT_B].rearrange("b (x c) t -> (b x) (c t)", c=8) for o in (out_0, out_1)]
 
-        def mx_passes(y, pos, hb):
+        def mx_passes(y, pos, h):
             cols = slice(P * order[pos], P * order[pos] + P)
             for i in range(4):
-                m = 4 * hb + i
+                m = 4 * h + i
                 nc.tensor.matmul_mx(out=y[:, i, :], lhsT=w_codes[:, m, :].bitcast(FP8X4), lhsT_scale=w_scales[:, m, :],
                                     rhs=x_codes[:, cols].bitcast(FP8X4), rhs_scale=x_scales[:, cols],
                                     start=True, stop=True)
 
-        def sums_mx(pos, hb):
+        def sums_mx(pos, h):
             if pos >= NCH:
                 return
-            ysum = ypsum.tile([P, 4, P], F32, name="ysum%d" % hb, tag="ysum%d" % hb)
-            mx_passes(ysum, pos, hb)
-            live[("ysum", hb)] = ysum
+            ysum = ypsum.tile([P, 4, P], F32, name="ysum%d" % h, tag="y%d" % h)
+            mx_passes(ysum, pos, h)
+            live[("ysum", h)] = ysum
 
-        def sums(pos, hb):
+        def sums(pos, h):
             if pos >= NCH:
                 return
             g, e = pos // 2, pos % 2
-            if e == 0 and hb == 0:
-                live[("s1", g)] = small.tile([P, 2, NM, 2], F32, name="s1", tag="s1")
+            if e == 0 and h == 0:
+                live[("s1", g)] = small.tile([P, 2, 2, 4, 2], F32, name="s1", tag="s1")
                 live[("acc", g)] = small.tile([P, 2, 2, 2], F32, name="acc", tag="acc")
             s1 = live[("s1", g)]
             acc = live[("acc", g)]
-            ysum = live[("ysum", hb)]
+            ysum = live[("ysum", h)]
             junk = small.tile([P, 4, T], F32)
-            nc.vector.tensor_reduce(out=s1[:, e, 4 * hb:4 * hb + 4, :].rearrange("p m l -> p (m l)"),
-                                    in_=ysum[:].rearrange("p m (l t) -> p (m l) t", l=2), axis=AX.X, op=ALU.add)
             for l in range(2):
                 nc.scalar.activation(out=junk[:], in_=ysum[:, :, T * l:T * l + T], func=ACT.Square,
-                                     accum_out=acc[:, e, hb, l:l + 1])
+                                     accum_out=acc[:, h, e, l:l + 1])
+            nc.vector.tensor_reduce(out=s1[:, h, e, :, :].rearrange("p i l -> p (i l)"),
+                                    in_=ysum[:].rearrange("p i (l t) -> p (i l) t", l=2), axis=AX.X, op=ALU.add)
 
         def chain_a(g):
             if g >= NCH // 2:
                 return
-            s1 = live[("s1", g)]
+            s1 = live[("s1", g)][:].rearrange("p h e i l -> p (h e) i l")
             acc = live[("acc", g)]
-            cross = small.tile([P, 2, NM, 2], F32)
-            nc.vector.tensor_tensor(out=cross[:], in0=s1[:],
-                                    in1=beta2[:].unsqueeze(1).unsqueeze(3).to_broadcast([P, 2, NM, 2]), op=ALU.mult)
-            rs = small.tile([P, 2, 2, 2], F32)
-            nc.vector.tensor_reduce(out=rs[:, 0, :, :], in_=s1[:].rearrange("p e m l -> p e l m"), axis=AX.X, op=ALU.add)
-            nc.vector.tensor_reduce(out=rs[:, 1, :, :], in_=cross[:].rearrange("p e m l -> p e l m"), axis=AX.X, op=ALU.add)
-            nc.vector.tensor_tensor(out=rs[:, 1, :, :], in0=rs[:, 1, :, :], in1=acc[:, :, 0, :], op=ALU.add)
-            nc.vector.tensor_tensor(out=rs[:, 1, :, :], in0=rs[:, 1, :, :], in1=acc[:, :, 1, :], op=ALU.add)
-            st = opsum.tile([P, 2, 4], F32, tag="op")
-            nc.tensor.matmul(out=st[:].rearrange("p s x -> p (s x)"), lhsT=bd2, rhs=rs[:].rearrange("p s e l -> p (s e l)"),
+            cross = small.tile([P, 4, 4, 2], F32)
+            nc.vector.tensor_tensor(out=cross[:], in0=s1, in1=beta2_w, op=ALU.mult)
+            rs = small.tile([P, 2, 4, 2], F32)
+            nc.vector.tensor_reduce(out=rs[:, 0, :, :], in_=s1.rearrange("p x i l -> p x l i"), axis=AX.X, op=ALU.add)
+            nc.vector.tensor_reduce(out=rs[:, 1, :, :], in_=cross[:].rearrange("p x i l -> p x l i"), axis=AX.X, op=ALU.add)
+            nc.vector.tensor_tensor(out=rs[:, 1, :, :], in0=rs[:, 1, :, :], in1=acc[:].rearrange("p h e l -> p (h e) l"), op=ALU.add)
+            st = opsum.tile([P, 4, 4], F32, tag="op")
+            nc.tensor.matmul(out=st[:].rearrange("p a b -> p (a b)"), lhsT=bd2, rhs=rs[:].rearrange("p s x l -> p (s x l)"),
                              start=True, stop=True)
             live[("st", g)] = st
 
@@ -242,13 +260,14 @@ def tile_coarsepyramid_pa_kernel(tc, feature, segments, w_lr, b_lr, g_lr, be_lr,
             if g >= NCH // 2:
                 return
             st = live[("st", g)]
-            mv = small.tile([P, 2, 4], F32)
-            nc.vector.tensor_tensor(out=mv[:], in0=st[:], in1=cg[:].unsqueeze(2).to_broadcast([P, 2, 4]), op=ALU.add)
-            var = small.tile([P, 4], F32)
+            mv = small.tile([P, 2, 8], F32)
+            nc.vector.tensor_tensor(out=mv[:].rearrange("p s (h x) -> p (s h) x", h=2), in0=st[:],
+                                    in1=cg[:].unsqueeze(2).to_broadcast([P, 4, 4]), op=ALU.add)
+            var = small.tile([P, 8], F32)
             nc.vector.tensor_tensor(out=var[:], in0=mv[:, 0, :], in1=mv[:, 0, :], op=ALU.mult)
             nc.vector.tensor_tensor(out=var[:], in0=mv[:, 1, :], in1=var[:], op=ALU.subtract)
             nc.vector.tensor_scalar(out=var[:], in0=var[:], scalar1=EPS, scalar2=None, op0=ALU.add)
-            std = small.tile([P, 4], F32)
+            std = small.tile([P, 8], F32)
             nc.scalar.activation(out=std[:], in_=var[:], func=ACT.Sqrt)
             live[("mv", g)] = mv
             live[("std", g)] = std
@@ -257,44 +276,45 @@ def tile_coarsepyramid_pa_kernel(tc, feature, segments, w_lr, b_lr, g_lr, be_lr,
             if g >= NCH // 2:
                 return
             mv = live[("mv", g)]
-            rstd = small.tile([P, 2, 2], F32)
-            nc.vector.reciprocal(out=rstd[:].rearrange("p e l -> p (e l)"), in_=live[("std", g)][:])
-            full = [P, 2, NM, 2]
+            rstd = small.tile([P, 4, 2], F32)
+            nc.vector.reciprocal(out=rstd[:].rearrange("p x l -> p (x l)"), in_=live[("std", g)][:])
+            full = [P, 4, 4, 2]
             sc = small.tile(full, F32)
-            nc.vector.tensor_tensor(out=sc[:], in0=gamma.unsqueeze(1).unsqueeze(3).to_broadcast(full),
-                                    in1=rstd[:].unsqueeze(2).to_broadcast(full), op=ALU.mult)
+            nc.vector.tensor_tensor(out=sc[:], in0=gamma_w, in1=rstd[:].unsqueeze(2).to_broadcast(full), op=ALU.mult)
             sh = small.tile(full, F32)
-            nc.vector.tensor_tensor(out=sh[:], in0=beta.unsqueeze(1).unsqueeze(3).to_broadcast(full),
-                                    in1=mv[:, 0, :].rearrange("p (e l) -> p e l", e=2).unsqueeze(2).to_broadcast(full),
+            nc.vector.tensor_tensor(out=sh[:], in0=beta_w,
+                                    in1=mv[:, 0, :].rearrange("p (x l) -> p x l", l=2).unsqueeze(2).to_broadcast(full),
                                     op=ALU.subtract)
             nc.vector.tensor_tensor(out=sh[:], in0=sh[:], in1=sc[:], op=ALU.mult)
-            nc.vector.tensor_tensor(out=sh[:], in0=sh[:], in1=shift0.unsqueeze(1).unsqueeze(3).to_broadcast(full), op=ALU.add)
+            nc.vector.tensor_tensor(out=sh[:], in0=sh[:], in1=shift_w, op=ALU.add)
             live[("sc", g)] = sc
             live[("sh", g)] = sh
 
         def main_mx(pos):
             ys = []
-            for hb in range(2):
-                y = ypsum.tile([P, 4, P], F32, name="y%d" % hb, tag="y%d" % hb)
-                mx_passes(y, pos, hb)
+            for h in range(2):
+                y = ypsum.tile([P, 4, P], F32, name="y%d" % h, tag="y%d" % h)
+                mx_passes(y, pos, h)
                 ys.append(y)
             live[("y", pos)] = ys
             live[("f", pos)] = fpool.tile([P, NM, P], F32, name="f", tag="f")
 
-        def apply_norm(pos, hb):
+        def apply_norm(pos, h):
             f = live[("f", pos)]
-            y = live[("y", pos)][hb]
+            y = live[("y", pos)][h]
             sc = live[("sc", pos // 2)]
             sh = live[("sh", pos // 2)]
-            e = pos % 2
+            x = 2 * h + pos % 2
             for i in range(4):
-                m = 4 * hb + i
                 for l in range(2):
-                    nc.scalar.activation(out=f[:, m, T * l:T * l + T], in_=y[:, i, T * l:T * l + T],
-                                         func=ACT.Relu, bias=sh[:, e, m, l:l + 1], scale=sc[:, e, m, l:l + 1])
+                    nc.scalar.activation(out=f[:, 4 * h + i, T * l:T * l + T], in_=y[:, i, T * l:T * l + T],
+                                         func=ACT.Relu, bias=sh[:, x, i, l:l + 1], scale=sc[:, x, i, l:l + 1])
 
-        def send(x, dst, src):
-            if held[x] is None:
+        def send(x, pos, tile_):
+            j = order[pos]
+            dst = (out_0, out_1)[x][2 * j:2 * j + 2].rearrange("l (h p i) t -> p (l h) (i t)", h=2, i=4)
+            src = tile_[:].rearrange("p l (h i) t -> p (l h) (i t)", h=2)
+            if j >= N_LATE or held[x] is None:
                 nc.sync.dma_start(out=dst, in_=src)
             else:
                 held[x].append((dst, src))
@@ -304,117 +324,107 @@ def tile_coarsepyramid_pa_kernel(tc, feature, segments, w_lr, b_lr, g_lr, be_lr,
                 nc.sync.dma_start(out=dst, in_=src)
             held[x] = None
 
+        def out_tile(pos, name):
+            if order[pos] < N_LATE:
+                return late.tile([P, 2, NM, T], F32, name=name + "_late", tag=name + "_late")
+            return opool.tile([P, 2, NM, T], F32, name=name, tag=name)
+
         def store_feat(pos):
-            j = order[pos]
-            is_late = j < SLOT_B // 2
-            f = live[("f", pos)]
-            if is_late:
-                f2 = late.tile([P, 2, NM, T], F32, name="f2_late", tag="f2_late")
-            else:
-                f2 = opool.tile([P, 2, NM, T], F32, name="f2", tag="f2")
-            nc.scalar.copy(out=f2[:], in_=f[:].rearrange("p m (l t) -> p l m t", l=2))
-            dst = out_0[2 * j:2 * j + 2].rearrange("l (p m) t -> p l (m t)", m=NM)
-            if is_late:
-                send(0, dst, f2[:].rearrange("p l m t -> p l (m t)"))
-            else:
-                nc.sync.dma_start(out=dst, in_=f2[:].rearrange("p l m t -> p l (m t)"))
+            f2 = out_tile(pos, "f2")
+            nc.scalar.copy(out=f2[:], in_=live[("f", pos)][:].rearrange("p m (l t) -> p l m t", l=2))
+            send(0, pos, f2)
+
+        def level(pos, k):
+            if k == 0:
+                return live[("f", pos)][:].rearrange("p m (l t) -> p m l t", l=2)
+            return tab[:, k - 1, :, 0:2 * L_STEP[k]].rearrange("p m (l t) -> p m l t", l=2)
 
         def level_up(pos, k):
             s = 2 ** k
             n_ok = T - 2 * s + 1
-            if k == 0:
-                prev = live[("f", pos)][:].rearrange("p m (l t) -> p (m l) t", l=2)
-            else:
-                prev = tab[:, k - 1, :, :].rearrange("p m (l t) -> p (m l) t", l=2)
-            nxt = tab[:, k, :, :].rearrange("p m (l t) -> p (m l) t", l=2)
-            nc.vector.tensor_tensor(out=nxt[:, :, 0:n_ok], in0=prev[:, :, 0:n_ok], in1=prev[:, :, s:s + n_ok], op=ALU.max)
+            prev = level(pos, k)
+            nc.vector.tensor_tensor(out=level(pos, k + 1)[:, :, :, 0:n_ok], in0=prev[:, :, :, 0:n_ok],
+                                    in1=prev[:, :, :, s:s + n_ok], op=ALU.max)
 
         def rows_out(pos, k):
-            f = live[("f", pos)]
             if k == 0:
-                live[("r", pos)] = rpool.tile([P, LEV, 2, NM, 64], F32, name="r", tag="r")
+                live[("r", pos)] = rpool.tile([P, LEV, 2, C], F32, name="r", tag="r")
             r = live[("r", pos)]
-            for hb in range(2):
+            for h in range(2):
                 tp = tpsum.tile([P, 4, P], F32, tag="tp")
                 for i in range(4):
-                    m = 4 * hb + i
-                    src = f[:, m, :] if k == 0 else tab[:, k - 1, m, :]
+                    m = 4 * h + i
+                    src = live[("f", pos)][:, m, :] if k == 0 else tab[:, k - 1, m, :]
                     nc.tensor.transpose(tp[:, i, :], src, ident[:])
-                dst = r[:, k, :, 4 * hb:4 * hb + 4, :]
-                view = tp[:].rearrange("p m (h q) -> p h m q", h=2)
-                if k >= 4:
-                    nc.vector.tensor_copy(out=dst, in_=view)
+                if 2 * k + h >= 7:
+                    nc.vector.tensor_copy(out=r[:, k, h, :], in_=tp[:].rearrange("p i q -> p (i q)"))
                 else:
-                    nc.scalar.copy(out=dst, in_=view)
-            if k % 2 == 1:
-                nc.sync.dma_start(out=slot_store[pos % 2][:, k - 1:k + 1, :],
-                                  in_=r[:, k - 1:k + 1, :, :, :].rearrange("p k h m q -> p k (h m q)"))
+                    nc.scalar.copy(out=r[:, k, h, :], in_=tp[:].rearrange("p i q -> p (i q)"))
+            slot = slot_wide[pos % 2]
+            if k in (1, 3):
+                nc.sync.dma_start(out=slot[ROW0[k - 1]:ROW0[k - 1] + 2 * P, :].rearrange("(k r) w -> r k w", k=2),
+                                  in_=r[:, k - 1:k + 1, :, :].rearrange("p k h c -> p k (h c)"))
+            if k >= 4:
+                n_r = 2 * L_STEP[k]
+                nc.sync.dma_start(out=slot[ROW0[k]:ROW0[k] + n_r, :], in_=r[0:n_r, k, :, :].rearrange("p h c -> p (h c)"))
 
         def gathers(pos):
             j = order[pos]
             got = []
             for h in range(2):
-                ga = gpool.tile([P, C], F32, name="ga%d" % h, tag="ga%d" % h, bufs=3)
-                gb = gpool.tile([P, C], F32, name="gb%d" % h, tag="gb%d" % h, bufs=3)
-                nc.gpsimd.indirect_dma_start(out=ga[:], out_offset=None, in_=slot_rows[pos % 2],
-                                             in_offset=bass.IndirectOffsetOnAxis(ap=idx[:, j, h, 0:1], axis=0))
-                nc.gpsimd.indirect_dma_start(out=gb[:], out_offset=None, in_=slot_rows[pos % 2],
-                                             in_offset=bass.IndirectOffsetOnAxis(ap=idx[:, j, h, 1:2], axis=0))
-                got.append((ga, gb))
+                pair = []
+                for e in range(2):
+                    ga = gpool.tile([P, C], F32, name="g%d%d" % (h, e), tag="g%d%d" % (h, e))
+                    nc.gpsimd.indirect_dma_start(out=ga[:], out_offset=None, in_=slot_rows[pos % 2],
+                                                 in_offset=bass.IndirectOffsetOnAxis(ap=idx[:, j, h, e:e + 1], axis=0))
+                    pair.append(ga)
+                got.append(pair)
             live[("g", pos)] = got
 
-        def window_max(pos):
-            gc = gpool.tile([P, NM, 2, 64], F32)
-            for h in range(2):
-                ga, gb = live[("g", pos)][h]
-                nc.vector.tensor_tensor(out=gc[:, :, h, :], in0=ga[:].rearrange("p (m q) -> p m q", m=NM),
-                                        in1=gb[:].rearrange("p (m q) -> p m q", m=NM), op=ALU.max)
-            live[("gc", pos)] = gc
+        def pooled_turn(pos, h):
+            banks = []
+            for e in range(2):
+                bank = opsum.tile([P, 4, P], F32, name="bank", tag="op")
+                for i in range(4):
+                    nc.tensor.transpose(bank[:, i, :], live[("g", pos)][h][e][:, P * i:P * i + P], ident[:])
+                banks.append(bank)
+                if e == 0:
+                    one = opool.tile([P, 4, P], F32, name="one", tag="one")
+                    nc.scalar.copy(out=one[:], in_=bank[:])
+            live[("turn", pos, h)] = (one, banks[1])
 
-        def pooled_out(pos, hb):
-            j = order[pos]
-            is_late = j < SLOT_B // 2
-            gc = live[("gc", pos)]
-            if hb == 0:
-                if is_late:
-                    live[("o", pos)] = late.tile([P, 2, NM, T], F32, name="o_late", tag="o_late")
-                else:
-                    live[("o", pos)] = opool.tile([P, 2, NM, T], F32, name="o", tag="o")
+        def pooled_max(pos, h):
+            if h == 0:
+                live[("o", pos)] = out_tile(pos, "o")
             o = live[("o", pos)]
-            op = opsum.tile([P, 4, P], F32, tag="op")
-            for i in range(4):
-                nc.tensor.transpose(op[:, i, :], gc[:, 4 * hb + i, :, :].rearrange("p h q -> p (h q)"), ident[:])
-            nc.scalar.copy(out=o[:, :, 4 * hb:4 * hb + 4, :], in_=op[:].rearrange("p m (l n) -> p l m n", l=2))
-            if hb == 1:
-                dst = out_1[2 * j:2 * j + 2].rearrange("l (p m) n -> p l (m n)", m=NM)
-                if is_late:
-                    send(1, dst, o[:].rearrange("p l m n -> p l (m n)"))
-                else:
-                    nc.sync.dma_start(out=dst, in_=o[:].rearrange("p l m n -> p l (m n)"))
+            one, bank = live[("turn", pos, h)]
+            nc.vector.tensor_tensor(out=o[:, :, 4 * h:4 * h + 4, :], in0=bank[:].rearrange("p i (l n) -> p l i n", l=2),
+                                    in1=one[:].rearrange("p i (l n) -> p l i n", l=2), op=ALU.max)
+            if h == 1:
+                send(1, pos, o)
 
         for pos in range(2):
-            for hb in range(2):
-                sums_mx(pos, hb)
-                sums(pos, hb)
+            for h in range(2):
+                sums_mx(pos, h)
+                sums(pos, h)
         chain_a(0)
         chain_b(0)
         chain_c(0)
-        for a in range(NCH + 4):
+        for a in range(NCH + 3):
             first = a < NCH
             second = 0 <= a - 1 < NCH
             third = 0 <= a - 3 < NCH
-            fourth = 0 <= a - 4 < NCH
             g_next = (a + 1) // 2 if a % 2 == 1 else NCH
             for q in range(2, len(pieces)):
                 if first_use(q) - 6 == a:
                     load_piece(q)
-            if fourth:
-                pooled_out(a - 4, 0)
             if second:
                 rows_out(a - 1, 0)
                 level_up(a - 1, 0)
             if first:
                 main_mx(a)
+            if third:
+                pooled_turn(a - 3, 0)
             if second:
                 level_up(a - 1, 1)
                 rows_out(a - 1, 1)
@@ -423,34 +433,36 @@ def tile_coarsepyramid_pa_kernel(tc, feature, segments, w_lr, b_lr, g_lr, be_lr,
                 apply_norm(a, 1)
                 store_feat(a)
                 quantise_piece(1)
-                for hb in range(2):
-                    sums_mx(2, hb)
-                    sums(2, hb)
+                for h in range(2):
+                    sums_mx(2, h)
+                    sums(2, h)
                 gather_indices()
-            sums_mx(a + 3, 0)
-            sums_mx(a + 3, 1)
             if second:
                 level_up(a - 1, 2)
                 rows_out(a - 1, 2)
                 level_up(a - 1, 3)
+            if third:
+                pooled_turn(a - 3, 1)
+            if second:
                 rows_out(a - 1, 3)
                 level_up(a - 1, 4)
                 rows_out(a - 1, 4)
                 rows_out(a - 1, 5)
                 gathers(a - 1)
+            if third:
+                pooled_max(a - 3, 0)
+                pooled_max(a - 3, 1)
+                if a - 3 >= NCH - 2:
+                    give_up_slot((a - 3) % 2)
             chain_a(g_next)
             if first and a > 0:
                 apply_norm(a, 0)
                 apply_norm(a, 1)
                 store_feat(a)
+            sums_mx(a + 3, 0)
+            sums_mx(a + 3, 1)
             sums(a + 3, 0)
             chain_b(g_next)
-            if third:
-                window_max(a - 3)
-                if a - 3 >= NCH - 2:
-                    give_up_slot((a - 3) % 2)
-            if fourth:
-                pooled_out(a - 4, 1)
             sums(a + 3, 1)
             chain_c(g_next)
             for q in range(2, len(pieces)):

@@ -20,26 +20,21 @@ NM = 8
 NCH = B // 2
 LEV = 6
 EPS = 1e-5
-L_STEP = [64, 64, 64, 64, 56, 40]
-ROW0 = [0, 128, 256, 384, 512, 624]
-N_ROWS = 704
-SLOT_B = 11
-N_LATE = 6
+SLOT_B = 12
 FLOPS = 2 * B * C2 * C * T
 
 
 def tile_coarsepyramid_pa_kernel(tc, feature, segments, w_lr, b_lr, g_lr, be_lr, out_0, out_1):
     nc = tc.nc
     with ExitStack() as ctx:
-        ctx.enter_context(tc.manual_schedule())
         const = ctx.enter_context(tc.tile_pool(name="const", bufs=1))
         small = ctx.enter_context(tc.tile_pool(name="small", bufs=3))
         stage = ctx.enter_context(tc.tile_pool(name="stage", bufs=2))
         ypsum = ctx.enter_context(tc.psum_pool(name="ypsum", bufs=1))
-        tpsum = ctx.enter_context(tc.psum_pool(name="tpsum", bufs=4))
-        opsum = ctx.enter_context(tc.psum_pool(name="opsum", bufs=2))
+        tpsum = ctx.enter_context(tc.psum_pool(name="tpsum", bufs=3))
+        opsum = ctx.enter_context(tc.psum_pool(name="opsum", bufs=1))
 
-        order = list(range(N_LATE, NCH)) + list(range(N_LATE))
+        order = list(range(SLOT_B // 2, NCH)) + list(range(SLOT_B // 2))
         live = {}
         held = {0: [], 1: []}
 
@@ -75,13 +70,11 @@ def tile_coarsepyramid_pa_kernel(tc, feature, segments, w_lr, b_lr, g_lr, be_lr,
         pid_i = const.tile([P, 1], I32)
         with tc.tile_pool(name="wstage", bufs=1) as wstage:
             w_sb = wstage.tile([P, NM, C], BF16)
-            nc.sync.dma_start(out=w_sb[:].rearrange("p (h i) k -> p h (i k)", h=2),
-                              in_=w_lr.rearrange("(h p i) k -> p h (i k)", h=2, i=4))
+            nc.sync.dma_start(out=w_sb[:], in_=w_lr.rearrange("(p m) k -> p m k", m=NM))
             load_piece(0)
             load_piece(1)
             for i, v in enumerate((b_lr, g_lr, be_lr)):
-                nc.scalar.dma_start(out=vec_bf[i][:].rearrange("p (h i) -> p h i", h=2),
-                                    in_=v.rearrange("(h p i) -> p h i", h=2, i=4))
+                nc.scalar.dma_start(out=vec_bf[i][:], in_=v.rearrange("(p m) -> p m", m=NM))
             nc.scalar.dma_start(out=seg_bf[:], in_=segments.rearrange("(j l) n s -> (l n) j s", l=2))
             make_identity(nc, ident[:])
             nc.gpsimd.iota(pid_i[:], pattern=[[0, 1]], base=0, channel_multiplier=1)
@@ -102,42 +95,36 @@ def tile_coarsepyramid_pa_kernel(tc, feature, segments, w_lr, b_lr, g_lr, be_lr,
                                   in_=w_grp[:].rearrange("p m c j -> p (m c j)"))
         quantise_piece(0)
 
-        grp = const.tile([P, 16], F32)
-        nc.vector.tensor_reduce(out=grp[:], in_=ident[:].rearrange("p (q r) -> p q r", r=8), axis=AX.X, op=ALU.add)
-        bd = const.tile([P, 16, 8], F32)
-        nc.vector.tensor_scalar(out=bd[:], in0=grp[:].unsqueeze(2).to_broadcast([P, 16, 8]),
+        grp = const.tile([P, 32], F32)
+        nc.vector.tensor_reduce(out=grp[:], in_=ident[:].rearrange("p (q r) -> p q r", r=4), axis=AX.X, op=ALU.add)
+        bd = const.tile([P, 32, 4], F32)
+        nc.vector.tensor_scalar(out=bd[:], in0=grp[:].unsqueeze(2).to_broadcast([P, 32, 4]),
                                 scalar1=1.0 / 2048.0, scalar2=None, op0=ALU.mult)
         bd2 = bd[:].rearrange("p q r -> p (q r)")
         vec = const.tile([P, 3, NM], F32)
         for i in range(3):
             nc.vector.tensor_copy(out=vec[:, i, :], in_=vec_bf[i][:])
-        wide = const.tile([P, 4, 2, 2, 4, 2], F32)
-        for i in range(3):
-            for e in range(2):
-                nc.vector.tensor_copy(out=wide[:, i, :, e, :, :],
-                                      in_=vec[:, i, :].rearrange("p (h i) -> p h i", h=2).unsqueeze(3).to_broadcast([P, 2, 4, 2]))
-        nc.vector.tensor_scalar(out=wide[:, 3, :, :, :, :].rearrange("p h e i l -> p (h e i l)"),
-                                in0=wide[:, 0, :, :, :, :].rearrange("p h e i l -> p (h e i l)"), scalar1=2.0, scalar2=None, op0=ALU.mult)
-        beta_w = wide[:, 0, :, :, :, :].rearrange("p h e i l -> p (h e) i l")
-        gamma_w = wide[:, 1, :, :, :, :].rearrange("p h e i l -> p (h e) i l")
-        shift_w = wide[:, 2, :, :, :, :].rearrange("p h e i l -> p (h e) i l")
-        beta2_w = wide[:, 3, :, :, :, :].rearrange("p h e i l -> p (h e) i l")
+        beta = vec[:, 0, :]
+        gamma = vec[:, 1, :]
+        shift0 = vec[:, 2, :]
+        beta2 = const.tile([P, NM], F32)
+        nc.vector.tensor_scalar(out=beta2[:], in0=beta, scalar1=2.0, scalar2=None, op0=ALU.mult)
         bsq = const.tile([P, NM], F32)
-        nc.vector.tensor_tensor(out=bsq[:], in0=vec[:, 0, :], in1=vec[:, 0, :], op=ALU.mult)
-        cc = const.tile([P, 2, 2], F32)
-        nc.vector.tensor_reduce(out=cc[:, 0, :], in_=vec[:, 0, :].rearrange("p (h i) -> p h i", h=2), axis=AX.X, op=ALU.add)
-        nc.vector.tensor_reduce(out=cc[:, 1, :], in_=bsq[:].rearrange("p (h i) -> p h i", h=2), axis=AX.X, op=ALU.add)
-        cc64 = const.tile([P, 4], F32)
-        nc.vector.tensor_scalar(out=cc64[:], in0=cc[:].rearrange("p s h -> p (s h)"), scalar1=64.0, scalar2=None, op0=ALU.mult)
-        cg_ps = opsum.tile([P, 4], F32, tag="op")
+        nc.vector.tensor_tensor(out=bsq[:], in0=beta, in1=beta, op=ALU.mult)
+        cc = const.tile([P, 2], F32)
+        nc.vector.tensor_reduce(out=cc[:, 0:1], in_=beta, axis=AX.X, op=ALU.add)
+        nc.vector.tensor_reduce(out=cc[:, 1:2], in_=bsq[:], axis=AX.X, op=ALU.add)
+        cc64 = const.tile([P, 2], F32)
+        nc.vector.tensor_scalar(out=cc64[:], in0=cc[:], scalar1=64.0, scalar2=None, op0=ALU.mult)
+        cg_ps = opsum.tile([P, 2], F32, tag="op")
         nc.tensor.matmul(out=cg_ps[:], lhsT=bd2, rhs=cc64[:], start=True, stop=True)
-        cg = const.tile([P, 4], F32)
+        cg = const.tile([P, 2], F32)
         nc.vector.tensor_copy(out=cg[:], in_=cg_ps[:])
 
         idx = const.tile([P, NCH, 2, 2], I32)
 
         def gather_indices():
-            nq = NCH * 2
+            NQ = NCH * 2
             sf = const.tile([P, NCH * 4], F32)
             nc.vector.tensor_copy(out=sf[:], in_=seg_bf[:].rearrange("p j s -> p (j s)"))
             nc.vector.tensor_scalar(out=sf[:], in0=sf[:], scalar1=0.0, scalar2=float(T - 1), op0=ALU.max, op1=ALU.min)
@@ -147,112 +134,106 @@ def tile_coarsepyramid_pa_kernel(tc, feature, segments, w_lr, b_lr, g_lr, be_lr,
             nc.vector.tensor_copy(out=sr[:], in_=si[:])
             over = const.tile([P, NCH * 4], F32)
             nc.vector.tensor_tensor(out=over[:], in0=sr[:], in1=sf[:], op=ALU.is_gt)
-            fl = const.tile([P, nq, 2], F32)
+            fl = const.tile([P, NQ, 2], F32)
             nc.vector.tensor_tensor(out=fl[:].rearrange("p q e -> p (q e)"), in0=sr[:], in1=over[:], op=ALU.subtract)
             lo = fl[:, :, 0]
             hi = fl[:, :, 1]
-            ln = const.tile([P, nq], F32)
+            ln = const.tile([P, NQ], F32)
             nc.vector.tensor_tensor(out=ln[:], in0=hi, in1=lo, op=ALU.subtract)
             nc.vector.tensor_scalar(out=ln[:], in0=ln[:], scalar1=1.0, scalar2=None, op0=ALU.add)
-            valid = const.tile([P, nq], F32)
+            valid = const.tile([P, NQ], F32)
             nc.vector.tensor_scalar(out=valid[:], in0=ln[:], scalar1=1.0, scalar2=None, op0=ALU.is_ge)
-            lev = const.tile([P, nq], F32)
-            wid = const.tile([P, nq], F32)
-            cut = const.tile([P, nq], F32)
-            for t_ in (lev, wid, cut):
-                nc.vector.memset(t_[:], 0.0)
-            step = const.tile([P, nq], F32)
+            lev256 = const.tile([P, NQ], F32)
+            wid = const.tile([P, NQ], F32)
+            nc.vector.memset(lev256[:], 0.0)
+            nc.vector.memset(wid[:], 0.0)
+            step = const.tile([P, NQ], F32)
             for k in range(1, LEV):
                 nc.vector.tensor_scalar(out=step[:], in0=ln[:], scalar1=float(2 ** k), scalar2=None, op0=ALU.is_ge)
-                nc.vector.scalar_tensor_tensor(out=lev[:], in0=step[:], scalar=float(2 * (ROW0[k] - ROW0[k - 1])), in1=lev[:],
-                                               op0=ALU.mult, op1=ALU.add)
-                nc.vector.scalar_tensor_tensor(out=wid[:], in0=step[:], scalar=float(2 ** (k - 1)), in1=wid[:],
-                                               op0=ALU.mult, op1=ALU.add)
-                if L_STEP[k] != L_STEP[k - 1]:
-                    nc.vector.scalar_tensor_tensor(out=cut[:], in0=step[:], scalar=float(2 * (L_STEP[k - 1] - L_STEP[k])),
-                                                   in1=cut[:], op0=ALU.mult, op1=ALU.add)
+                nc.vector.scalar_tensor_tensor(out=lev256[:], in0=step[:], scalar=256.0, in1=lev256[:], op0=ALU.mult, op1=ALU.add)
+                nc.vector.scalar_tensor_tensor(out=wid[:], in0=step[:], scalar=float(2 ** (k - 1)), in1=wid[:], op0=ALU.mult, op1=ALU.add)
             low_i = const.tile([P, 1], I32)
-            nc.vector.tensor_single_scalar(out=low_i[:], in_=pid_i[:], scalar=3, op=ALU.bitwise_and)
+            nc.vector.tensor_single_scalar(out=low_i[:], in_=pid_i[:], scalar=15, op=ALU.bitwise_and)
             pid = const.tile([P, 1], F32)
             nc.vector.tensor_copy(out=pid[:], in_=pid_i[:])
             low = const.tile([P, 1], F32)
             nc.vector.tensor_copy(out=low[:], in_=low_i[:])
-            l_neg = const.tile([P, 1], F32)
-            nc.vector.tensor_scalar(out=l_neg[:], in0=pid[:], scalar1=64.0, scalar2=-1.0, op0=ALU.is_ge, op1=ALU.mult)
-            z0 = const.tile([P, 1], F32)
-            nc.vector.tensor_scalar(out=z0[:], in0=low[:], scalar1=2.0, scalar2=float(2 * (ROW0[5] + 33)), op0=ALU.mult, op1=ALU.add)
+            lbase = const.tile([P, 1], F32)
+            nc.vector.tensor_scalar(out=lbase[:], in0=pid[:], scalar1=64.0, scalar2=128.0, op0=ALU.is_ge, op1=ALU.mult)
             zrow = const.tile([P, 1], F32)
-            nc.vector.scalar_tensor_tensor(out=zrow[:], in0=l_neg[:], scalar=float(-2 * L_STEP[5]), in1=z0[:], op0=ALU.mult, op1=ALU.add)
-            zrel = const.tile([P, 1], F32)
-            nc.vector.scalar_tensor_tensor(out=zrel[:], in0=l_neg[:], scalar=128.0, in1=zrow[:], op0=ALU.mult, op1=ALU.add)
-            nc.vector.scalar_tensor_tensor(out=lev[:], in0=cut[:], scalar=l_neg[:, 0:1], in1=lev[:], op0=ALU.mult, op1=ALU.add)
-            rows = const.tile([P, nq, 2], F32)
-            nc.vector.scalar_tensor_tensor(out=rows[:, :, 0], in0=lo, scalar=2.0, in1=lev[:], op0=ALU.mult, op1=ALU.add)
-            t2 = const.tile([P, nq], F32)
+            nc.vector.tensor_scalar(out=zrow[:], in0=low[:], scalar1=2.0, scalar2=float(5 * 256 + 2 * 48), op0=ALU.mult, op1=ALU.add)
+            rows = const.tile([P, NQ, 2], F32)
+            nc.vector.scalar_tensor_tensor(out=rows[:, :, 0], in0=lo, scalar=2.0, in1=lev256[:], op0=ALU.mult, op1=ALU.add)
+            t2 = const.tile([P, NQ], F32)
             nc.vector.tensor_tensor(out=t2[:], in0=hi, in1=wid[:], op=ALU.subtract)
-            nc.vector.scalar_tensor_tensor(out=rows[:, :, 1], in0=t2[:], scalar=2.0, in1=lev[:], op0=ALU.mult, op1=ALU.add)
+            nc.vector.scalar_tensor_tensor(out=rows[:, :, 1], in0=t2[:], scalar=2.0, in1=lev256[:], op0=ALU.mult, op1=ALU.add)
             for e in range(2):
-                nc.vector.tensor_scalar(out=rows[:, :, e], in0=rows[:, :, e], scalar1=zrel[:, 0:1], scalar2=None, op0=ALU.subtract)
+                nc.vector.tensor_scalar(out=rows[:, :, e], in0=rows[:, :, e], scalar1=zrow[:, 0:1], scalar2=None, op0=ALU.subtract)
                 nc.vector.tensor_tensor(out=rows[:, :, e], in0=rows[:, :, e], in1=valid[:], op=ALU.mult)
-                nc.vector.tensor_scalar(out=rows[:, :, e], in0=rows[:, :, e], scalar1=zrow[:, 0:1], scalar2=None, op0=ALU.add)
+                nc.vector.tensor_scalar(out=rows[:, :, e], in0=rows[:, :, e], scalar1=zrow[:, 0:1], scalar2=lbase[:, 0:1], op0=ALU.add, op1=ALU.add)
             rows4 = rows[:].rearrange("p (j h) e -> p j h e", h=2)
             nc.vector.tensor_scalar(out=rows4[:, :, 1, :], in0=rows4[:, :, 1, :], scalar1=1.0, scalar2=None, op0=ALU.add)
             nc.vector.tensor_copy(out=idx[:].rearrange("p j h e -> p (j h e)"), in_=rows[:].rearrange("p q e -> p (q e)"))
 
+
         fpool = ctx.enter_context(tc.tile_pool(name="fpool", bufs=2))
-        late = ctx.enter_context(tc.tile_pool(name="late", bufs=N_LATE))
+        late = ctx.enter_context(tc.tile_pool(name="late", bufs=6))
         rpool = ctx.enter_context(tc.tile_pool(name="rpool", bufs=2))
-        gpool = ctx.enter_context(tc.tile_pool(name="gpool", bufs=3))
+        gpool = ctx.enter_context(tc.tile_pool(name="gpool", bufs=2))
         opool = ctx.enter_context(tc.tile_pool(name="opool", bufs=2))
 
-        slot_wide = [o[0:SLOT_B].rearrange("b (x c) t -> (b x) (c t)", c=16) for o in (out_0, out_1)]
-        slot_rows = [o[0:SLOT_B].rearrange("b (x c) t -> (b x) (c t)", c=8) for o in (out_0, out_1)]
+        slots = [out_0, out_1]
+        slot_store = [o[0:SLOT_B].rearrange("b (x c) t -> (b x) (c t)", c=16).rearrange("(k r) w -> r k w", k=LEV)
+                      for o in slots]
+        slot_rows = [o[0:SLOT_B].rearrange("b (x c) t -> (b x) (c t)", c=8) for o in slots]
 
-        def mx_passes(y, pos, h):
+        def mx_passes(y, pos, hb):
             cols = slice(P * order[pos], P * order[pos] + P)
             for i in range(4):
-                m = 4 * h + i
+                m = 4 * hb + i
                 nc.tensor.matmul_mx(out=y[:, i, :], lhsT=w_codes[:, m, :].bitcast(FP8X4), lhsT_scale=w_scales[:, m, :],
                                     rhs=x_codes[:, cols].bitcast(FP8X4), rhs_scale=x_scales[:, cols],
                                     start=True, stop=True)
 
-        def sums_mx(pos, h):
+        def sums_mx(pos, hb):
             if pos >= NCH:
                 return
-            ysum = ypsum.tile([P, 4, P], F32, name="ysum%d" % h, tag="y%d" % h)
-            mx_passes(ysum, pos, h)
-            live[("ysum", h)] = ysum
+            ysum = ypsum.tile([P, 4, P], F32, name="ysum%d" % hb, tag="ysum%d" % hb)
+            mx_passes(ysum, pos, hb)
+            live[("ysum", hb)] = ysum
 
-        def sums(pos, h):
+        def sums(pos, hb):
             if pos >= NCH:
                 return
             g, e = pos // 2, pos % 2
-            if e == 0 and h == 0:
-                live[("s1", g)] = small.tile([P, 2, 2, 4, 2], F32, name="s1", tag="s1")
+            if e == 0 and hb == 0:
+                live[("s1", g)] = small.tile([P, 2, NM, 2], F32, name="s1", tag="s1")
                 live[("acc", g)] = small.tile([P, 2, 2, 2], F32, name="acc", tag="acc")
             s1 = live[("s1", g)]
             acc = live[("acc", g)]
-            ysum = live[("ysum", h)]
+            ysum = live[("ysum", hb)]
             junk = small.tile([P, 4, T], F32)
+            nc.vector.tensor_reduce(out=s1[:, e, 4 * hb:4 * hb + 4, :].rearrange("p m l -> p (m l)"),
+                                    in_=ysum[:].rearrange("p m (l t) -> p (m l) t", l=2), axis=AX.X, op=ALU.add)
             for l in range(2):
                 nc.scalar.activation(out=junk[:], in_=ysum[:, :, T * l:T * l + T], func=ACT.Square,
-                                     accum_out=acc[:, h, e, l:l + 1])
-            nc.vector.tensor_reduce(out=s1[:, h, e, :, :].rearrange("p i l -> p (i l)"),
-                                    in_=ysum[:].rearrange("p i (l t) -> p (i l) t", l=2), axis=AX.X, op=ALU.add)
+                                     accum_out=acc[:, e, hb, l:l + 1])
 
         def chain_a(g):
             if g >= NCH // 2:
                 return
-            s1 = live[("s1", g)][:].rearrange("p h e i l -> p (h e) i l")
+            s1 = live[("s1", g)]
             acc = live[("acc", g)]
-            cross = small.tile([P, 4, 4, 2], F32)
-            nc.vector.tensor_tensor(out=cross[:], in0=s1, in1=beta2_w, op=ALU.mult)
-            rs = small.tile([P, 2, 4, 2], F32)
-            nc.vector.tensor_reduce(out=rs[:, 0, :, :], in_=s1.rearrange("p x i l -> p x l i"), axis=AX.X, op=ALU.add)
-            nc.vector.tensor_reduce(out=rs[:, 1, :, :], in_=cross[:].rearrange("p x i l -> p x l i"), axis=AX.X, op=ALU.add)
-            nc.vector.tensor_tensor(out=rs[:, 1, :, :], in0=rs[:, 1, :, :], in1=acc[:].rearrange("p h e l -> p (h e) l"), op=ALU.add)
-            st = opsum.tile([P, 4, 4], F32, tag="op")
-            nc.tensor.matmul(out=st[:].rearrange("p a b -> p (a b)"), lhsT=bd2, rhs=rs[:].rearrange("p s x l -> p (s x l)"),
+            cross = small.tile([P, 2, NM, 2], F32)
+            nc.vector.tensor_tensor(out=cross[:], in0=s1[:],
+                                    in1=beta2[:].unsqueeze(1).unsqueeze(3).to_broadcast([P, 2, NM, 2]), op=ALU.mult)
+            rs = small.tile([P, 2, 2, 2], F32)
+            nc.vector.tensor_reduce(out=rs[:, 0, :, :], in_=s1[:].rearrange("p e m l -> p e l m"), axis=AX.X, op=ALU.add)
+            nc.vector.tensor_reduce(out=rs[:, 1, :, :], in_=cross[:].rearrange("p e m l -> p e l m"), axis=AX.X, op=ALU.add)
+            nc.vector.tensor_tensor(out=rs[:, 1, :, :], in0=rs[:, 1, :, :], in1=acc[:, :, 0, :], op=ALU.add)
+            nc.vector.tensor_tensor(out=rs[:, 1, :, :], in0=rs[:, 1, :, :], in1=acc[:, :, 1, :], op=ALU.add)
+            st = opsum.tile([P, 2, 4], F32, tag="op")
+            nc.tensor.matmul(out=st[:].rearrange("p s x -> p (s x)"), lhsT=bd2, rhs=rs[:].rearrange("p s e l -> p (s e l)"),
                              start=True, stop=True)
             live[("st", g)] = st
 
@@ -260,14 +241,13 @@ def tile_coarsepyramid_pa_kernel(tc, feature, segments, w_lr, b_lr, g_lr, be_lr,
             if g >= NCH // 2:
                 return
             st = live[("st", g)]
-            mv = small.tile([P, 2, 8], F32)
-            nc.vector.tensor_tensor(out=mv[:].rearrange("p s (h x) -> p (s h) x", h=2), in0=st[:],
-                                    in1=cg[:].unsqueeze(2).to_broadcast([P, 4, 4]), op=ALU.add)
-            var = small.tile([P, 8], F32)
+            mv = small.tile([P, 2, 4], F32)
+            nc.vector.tensor_tensor(out=mv[:], in0=st[:], in1=cg[:].unsqueeze(2).to_broadcast([P, 2, 4]), op=ALU.add)
+            var = small.tile([P, 4], F32)
             nc.vector.tensor_tensor(out=var[:], in0=mv[:, 0, :], in1=mv[:, 0, :], op=ALU.mult)
             nc.vector.tensor_tensor(out=var[:], in0=mv[:, 1, :], in1=var[:], op=ALU.subtract)
             nc.vector.tensor_scalar(out=var[:], in0=var[:], scalar1=EPS, scalar2=None, op0=ALU.add)
-            std = small.tile([P, 8], F32)
+            std = small.tile([P, 4], F32)
             nc.scalar.activation(out=std[:], in_=var[:], func=ACT.Sqrt)
             live[("mv", g)] = mv
             live[("std", g)] = std
@@ -276,45 +256,44 @@ def tile_coarsepyramid_pa_kernel(tc, feature, segments, w_lr, b_lr, g_lr, be_lr,
             if g >= NCH // 2:
                 return
             mv = live[("mv", g)]
-            rstd = small.tile([P, 4, 2], F32)
-            nc.vector.reciprocal(out=rstd[:].rearrange("p x l -> p (x l)"), in_=live[("std", g)][:])
-            full = [P, 4, 4, 2]
+            rstd = small.tile([P, 2, 2], F32)
+            nc.vector.reciprocal(out=rstd[:].rearrange("p e l -> p (e l)"), in_=live[("std", g)][:])
+            full = [P, 2, NM, 2]
             sc = small.tile(full, F32)
-            nc.vector.tensor_tensor(out=sc[:], in0=gamma_w, in1=rstd[:].unsqueeze(2).to_broadcast(full), op=ALU.mult)
+            nc.vector.tensor_tensor(out=sc[:], in0=gamma.unsqueeze(1).unsqueeze(3).to_broadcast(full),
+                                    in1=rstd[:].unsqueeze(2).to_broadcast(full), op=ALU.mult)
             sh = small.tile(full, F32)
-            nc.vector.tensor_tensor(out=sh[:], in0=beta_w,
-                                    in1=mv[:, 0, :].rearrange("p (x l) -> p x l", l=2).unsqueeze(2).to_broadcast(full),
+            nc.vector.tensor_tensor(out=sh[:], in0=beta.unsqueeze(1).unsqueeze(3).to_broadcast(full),
+                                    in1=mv[:, 0, :].rearrange("p (e l) -> p e l", e=2).unsqueeze(2).to_broadcast(full),
                                     op=ALU.subtract)
             nc.vector.tensor_tensor(out=sh[:], in0=sh[:], in1=sc[:], op=ALU.mult)
-            nc.vector.tensor_tensor(out=sh[:], in0=sh[:], in1=shift_w, op=ALU.add)
+            nc.vector.tensor_tensor(out=sh[:], in0=sh[:], in1=shift0.unsqueeze(1).unsqueeze(3).to_broadcast(full), op=ALU.add)
             live[("sc", g)] = sc
             live[("sh", g)] = sh
 
         def main_mx(pos):
             ys = []
-            for h in range(2):
-                y = ypsum.tile([P, 4, P], F32, name="y%d" % h, tag="y%d" % h)
-                mx_passes(y, pos, h)
+            for hb in range(2):
+                y = ypsum.tile([P, 4, P], F32, name="y%d" % hb, tag="y%d" % hb)
+                mx_passes(y, pos, hb)
                 ys.append(y)
             live[("y", pos)] = ys
             live[("f", pos)] = fpool.tile([P, NM, P], F32, name="f", tag="f")
 
-        def apply_norm(pos, h):
+        def apply_norm(pos, hb):
             f = live[("f", pos)]
-            y = live[("y", pos)][h]
+            y = live[("y", pos)][hb]
             sc = live[("sc", pos // 2)]
             sh = live[("sh", pos // 2)]
-            x = 2 * h + pos % 2
+            e = pos % 2
             for i in range(4):
+                m = 4 * hb + i
                 for l in range(2):
-                    nc.scalar.activation(out=f[:, 4 * h + i, T * l:T * l + T], in_=y[:, i, T * l:T * l + T],
-                                         func=ACT.Relu, bias=sh[:, x, i, l:l + 1], scale=sc[:, x, i, l:l + 1])
+                    nc.scalar.activation(out=f[:, m, T * l:T * l + T], in_=y[:, i, T * l:T * l + T],
+                                         func=ACT.Relu, bias=sh[:, e, m, l:l + 1], scale=sc[:, e, m, l:l + 1])
 
-        def send(x, pos, tile_):
-            j = order[pos]
-            dst = (out_0, out_1)[x][2 * j:2 * j + 2].rearrange("l (h p i) t -> p (l h) (i t)", h=2, i=4)
-            src = tile_[:].rearrange("p l (h i) t -> p (l h) (i t)", h=2)
-            if j >= N_LATE or held[x] is None:
+        def send(x, dst, src):
+            if held[x] is None:
                 nc.sync.dma_start(out=dst, in_=src)
             else:
                 held[x].append((dst, src))
@@ -324,107 +303,117 @@ def tile_coarsepyramid_pa_kernel(tc, feature, segments, w_lr, b_lr, g_lr, be_lr,
                 nc.sync.dma_start(out=dst, in_=src)
             held[x] = None
 
-        def out_tile(pos, name):
-            if order[pos] < N_LATE:
-                return late.tile([P, 2, NM, T], F32, name=name + "_late", tag=name + "_late")
-            return opool.tile([P, 2, NM, T], F32, name=name, tag=name)
-
         def store_feat(pos):
-            f2 = out_tile(pos, "f2")
-            nc.scalar.copy(out=f2[:], in_=live[("f", pos)][:].rearrange("p m (l t) -> p l m t", l=2))
-            send(0, pos, f2)
-
-        def level(pos, k):
-            if k == 0:
-                return live[("f", pos)][:].rearrange("p m (l t) -> p m l t", l=2)
-            return tab[:, k - 1, :, 0:2 * L_STEP[k]].rearrange("p m (l t) -> p m l t", l=2)
+            j = order[pos]
+            is_late = j < SLOT_B // 2
+            f = live[("f", pos)]
+            if is_late:
+                f2 = late.tile([P, 2, NM, T], F32, name="f2_late", tag="f2_late")
+            else:
+                f2 = opool.tile([P, 2, NM, T], F32, name="f2", tag="f2")
+            nc.scalar.copy(out=f2[:], in_=f[:].rearrange("p m (l t) -> p l m t", l=2))
+            dst = out_0[2 * j:2 * j + 2].rearrange("l (p m) t -> p l (m t)", m=NM)
+            if is_late:
+                send(0, dst, f2[:].rearrange("p l m t -> p l (m t)"))
+            else:
+                nc.sync.dma_start(out=dst, in_=f2[:].rearrange("p l m t -> p l (m t)"))
 
         def level_up(pos, k):
             s = 2 ** k
             n_ok = T - 2 * s + 1
-            prev = level(pos, k)
-            nc.vector.tensor_tensor(out=level(pos, k + 1)[:, :, :, 0:n_ok], in0=prev[:, :, :, 0:n_ok],
-                                    in1=prev[:, :, :, s:s + n_ok], op=ALU.max)
+            if k == 0:
+                prev = live[("f", pos)][:].rearrange("p m (l t) -> p (m l) t", l=2)
+            else:
+                prev = tab[:, k - 1, :, :].rearrange("p m (l t) -> p (m l) t", l=2)
+            nxt = tab[:, k, :, :].rearrange("p m (l t) -> p (m l) t", l=2)
+            nc.vector.tensor_tensor(out=nxt[:, :, 0:n_ok], in0=prev[:, :, 0:n_ok], in1=prev[:, :, s:s + n_ok], op=ALU.max)
 
         def rows_out(pos, k):
+            f = live[("f", pos)]
             if k == 0:
-                live[("r", pos)] = rpool.tile([P, LEV, 2, C], F32, name="r", tag="r")
+                live[("r", pos)] = rpool.tile([P, LEV, 2, NM, 64], F32, name="r", tag="r")
             r = live[("r", pos)]
-            for h in range(2):
+            for hb in range(2):
                 tp = tpsum.tile([P, 4, P], F32, tag="tp")
                 for i in range(4):
-                    m = 4 * h + i
-                    src = live[("f", pos)][:, m, :] if k == 0 else tab[:, k - 1, m, :]
+                    m = 4 * hb + i
+                    src = f[:, m, :] if k == 0 else tab[:, k - 1, m, :]
                     nc.tensor.transpose(tp[:, i, :], src, ident[:])
-                if 2 * k + h >= 7:
-                    nc.vector.tensor_copy(out=r[:, k, h, :], in_=tp[:].rearrange("p i q -> p (i q)"))
+                dst = r[:, k, :, 4 * hb:4 * hb + 4, :]
+                view = tp[:].rearrange("p m (h q) -> p h m q", h=2)
+                if k >= 4:
+                    nc.vector.tensor_copy(out=dst, in_=view)
                 else:
-                    nc.scalar.copy(out=r[:, k, h, :], in_=tp[:].rearrange("p i q -> p (i q)"))
-            slot = slot_wide[pos % 2]
-            if k in (1, 3):
-                nc.sync.dma_start(out=slot[ROW0[k - 1]:ROW0[k - 1] + 2 * P, :].rearrange("(k r) w -> r k w", k=2),
-                                  in_=r[:, k - 1:k + 1, :, :].rearrange("p k h c -> p k (h c)"))
-            if k >= 4:
-                n_r = 2 * L_STEP[k]
-                nc.sync.dma_start(out=slot[ROW0[k]:ROW0[k] + n_r, :], in_=r[0:n_r, k, :, :].rearrange("p h c -> p (h c)"))
+                    nc.scalar.copy(out=dst, in_=view)
+            if k % 2 == 1:
+                nc.sync.dma_start(out=slot_store[pos % 2][:, k - 1:k + 1, :],
+                                  in_=r[:, k - 1:k + 1, :, :, :].rearrange("p k h m q -> p k (h m q)"))
 
         def gathers(pos):
             j = order[pos]
             got = []
             for h in range(2):
-                pair = []
-                for e in range(2):
-                    ga = gpool.tile([P, C], F32, name="g%d%d" % (h, e), tag="g%d%d" % (h, e))
-                    nc.gpsimd.indirect_dma_start(out=ga[:], out_offset=None, in_=slot_rows[pos % 2],
-                                                 in_offset=bass.IndirectOffsetOnAxis(ap=idx[:, j, h, e:e + 1], axis=0))
-                    pair.append(ga)
-                got.append(pair)
+                ga = gpool.tile([P, C], F32, name="ga%d" % h, tag="ga%d" % h, bufs=3)
+                gb = gpool.tile([P, C], F32, name="gb%d" % h, tag="gb%d" % h, bufs=3)
+                nc.gpsimd.indirect_dma_start(out=ga[:], out_offset=None, in_=slot_rows[pos % 2],
+                                             in_offset=bass.IndirectOffsetOnAxis(ap=idx[:, j, h, 0:1], axis=0))
+                nc.gpsimd.indirect_dma_start(out=gb[:], out_offset=None, in_=slot_rows[pos % 2],
+                                             in_offset=bass.IndirectOffsetOnAxis(ap=idx[:, j, h, 1:2], axis=0))
+                got.append((ga, gb))
             live[("g", pos)] = got
 
-        def pooled_turn(pos, h):
-            banks = []
-            for e in range(2):
-                bank = opsum.tile([P, 4, P], F32, name="bank", tag="op")
-                for i in range(4):
-                    nc.tensor.transpose(bank[:, i, :], live[("g", pos)][h][e][:, P * i:P * i + P], ident[:])
-                banks.append(bank)
-                if e == 0:
-                    one = opool.tile([P, 4, P], F32, name="one", tag="one")
-                    nc.scalar.copy(out=one[:], in_=bank[:])
-            live[("turn", pos, h)] = (one, banks[1])
+        def window_max(pos):
+            gc = gpool.tile([P, NM, 2, 64], F32)
+            for h in range(2):
+                ga, gb = live[("g", pos)][h]
+                nc.vector.tensor_tensor(out=gc[:, :, h, :], in0=ga[:].rearrange("p (m q) -> p m q", m=NM),
+                                        in1=gb[:].rearrange("p (m q) -> p m q", m=NM), op=ALU.max)
+            live[("gc", pos)] = gc
 
-        def pooled_max(pos, h):
-            if h == 0:
-                live[("o", pos)] = out_tile(pos, "o")
+        def pooled_out(pos, hb):
+            j = order[pos]
+            is_late = j < SLOT_B // 2
+            gc = live[("gc", pos)]
+            if hb == 0:
+                if is_late:
+                    live[("o", pos)] = late.tile([P, 2, NM, T], F32, name="o_late", tag="o_late")
+                else:
+                    live[("o", pos)] = opool.tile([P, 2, NM, T], F32, name="o", tag="o")
             o = live[("o", pos)]
-            one, bank = live[("turn", pos, h)]
-            nc.vector.tensor_tensor(out=o[:, :, 4 * h:4 * h + 4, :], in0=bank[:].rearrange("p i (l n) -> p l i n", l=2),
-                                    in1=one[:].rearrange("p i (l n) -> p l i n", l=2), op=ALU.max)
-            if h == 1:
-                send(1, pos, o)
+            op = opsum.tile([P, 4, P], F32, tag="op")
+            for i in range(4):
+                nc.tensor.transpose(op[:, i, :], gc[:, 4 * hb + i, :, :].rearrange("p h q -> p (h q)"), ident[:])
+            nc.scalar.copy(out=o[:, :, 4 * hb:4 * hb + 4, :], in_=op[:].rearrange("p m (l n) -> p l m n", l=2))
+            if hb == 1:
+                dst = out_1[2 * j:2 * j + 2].rearrange("l (p m) n -> p l (m n)", m=NM)
+                if is_late:
+                    send(1, dst, o[:].rearrange("p l m n -> p l (m n)"))
+                else:
+                    nc.sync.dma_start(out=dst, in_=o[:].rearrange("p l m n -> p l (m n)"))
 
         for pos in range(2):
-            for h in range(2):
-                sums_mx(pos, h)
-                sums(pos, h)
+            for hb in range(2):
+                sums_mx(pos, hb)
+                sums(pos, hb)
         chain_a(0)
         chain_b(0)
         chain_c(0)
-        for a in range(NCH + 3):
+        for a in range(NCH + 4):
             first = a < NCH
             second = 0 <= a - 1 < NCH
             third = 0 <= a - 3 < NCH
+            fourth = 0 <= a - 4 < NCH
             g_next = (a + 1) // 2 if a % 2 == 1 else NCH
             for q in range(2, len(pieces)):
                 if first_use(q) - 6 == a:
                     load_piece(q)
+            if fourth:
+                pooled_out(a - 4, 0)
             if second:
                 rows_out(a - 1, 0)
                 level_up(a - 1, 0)
             if first:
                 main_mx(a)
-            if third:
-                pooled_turn(a - 3, 0)
             if second:
                 level_up(a - 1, 1)
                 rows_out(a - 1, 1)
@@ -433,36 +422,34 @@ def tile_coarsepyramid_pa_kernel(tc, feature, segments, w_lr, b_lr, g_lr, be_lr,
                 apply_norm(a, 1)
                 store_feat(a)
                 quantise_piece(1)
-                for h in range(2):
-                    sums_mx(2, h)
-                    sums(2, h)
+                for hb in range(2):
+                    sums_mx(2, hb)
+                    sums(2, hb)
                 gather_indices()
+            sums_mx(a + 3, 0)
+            sums_mx(a + 3, 1)
             if second:
                 level_up(a - 1, 2)
                 rows_out(a - 1, 2)
                 level_up(a - 1, 3)
-            if third:
-                pooled_turn(a - 3, 1)
-            if second:
                 rows_out(a - 1, 3)
                 level_up(a - 1, 4)
                 rows_out(a - 1, 4)
                 rows_out(a - 1, 5)
                 gathers(a - 1)
-            if third:
-                pooled_max(a - 3, 0)
-                pooled_max(a - 3, 1)
-                if a - 3 >= NCH - 2:
-                    give_up_slot((a - 3) % 2)
             chain_a(g_next)
             if first and a > 0:
                 apply_norm(a, 0)
                 apply_norm(a, 1)
                 store_feat(a)
-            sums_mx(a + 3, 0)
-            sums_mx(a + 3, 1)
             sums(a + 3, 0)
             chain_b(g_next)
+            if third:
+                window_max(a - 3)
+                if a - 3 >= NCH - 2:
+                    give_up_slot((a - 3) % 2)
+            if fourth:
+                pooled_out(a - 4, 1)
             sums(a + 3, 1)
             chain_c(g_next)
             for q in range(2, len(pieces)):

@@ -20,7 +20,11 @@ NM = 8
 NCH = B // 2
 LEV = 6
 EPS = 1e-5
-SLOT_B = 12
+L_STEP = [64, 64, 64, 64, 56, 40]
+ROW0 = [0, 128, 256, 384, 512, 624]
+N_ROWS = 704
+SLOT_B = 11
+N_LATE = 6
 FLOPS = 2 * B * C2 * C * T
 
 
@@ -31,10 +35,10 @@ def tile_coarsepyramid_pa_kernel(tc, feature, segments, w_lr, b_lr, g_lr, be_lr,
         small = ctx.enter_context(tc.tile_pool(name="small", bufs=3))
         stage = ctx.enter_context(tc.tile_pool(name="stage", bufs=2))
         ypsum = ctx.enter_context(tc.psum_pool(name="ypsum", bufs=1))
-        tpsum = ctx.enter_context(tc.psum_pool(name="tpsum", bufs=3))
-        opsum = ctx.enter_context(tc.psum_pool(name="opsum", bufs=1))
+        tpsum = ctx.enter_context(tc.psum_pool(name="tpsum", bufs=4))
+        opsum = ctx.enter_context(tc.psum_pool(name="opsum", bufs=2))
 
-        order = list(range(SLOT_B // 2, NCH)) + list(range(SLOT_B // 2))
+        order = list(range(N_LATE, NCH)) + list(range(N_LATE))
         live = {}
         held = {0: [], 1: []}
 
@@ -70,11 +74,13 @@ def tile_coarsepyramid_pa_kernel(tc, feature, segments, w_lr, b_lr, g_lr, be_lr,
         pid_i = const.tile([P, 1], I32)
         with tc.tile_pool(name="wstage", bufs=1) as wstage:
             w_sb = wstage.tile([P, NM, C], BF16)
-            nc.sync.dma_start(out=w_sb[:], in_=w_lr.rearrange("(p m) k -> p m k", m=NM))
+            nc.sync.dma_start(out=w_sb[:].rearrange("p (h i) k -> p h (i k)", h=2),
+                              in_=w_lr.rearrange("(h p i) k -> p h (i k)", h=2, i=4))
             load_piece(0)
             load_piece(1)
             for i, v in enumerate((b_lr, g_lr, be_lr)):
-                nc.scalar.dma_start(out=vec_bf[i][:], in_=v.rearrange("(p m) -> p m", m=NM))
+                nc.scalar.dma_start(out=vec_bf[i][:].rearrange("p (h i) -> p h i", h=2),
+                                    in_=v.rearrange("(h p i) -> p h i", h=2, i=4))
             nc.scalar.dma_start(out=seg_bf[:], in_=segments.rearrange("(j l) n s -> (l n) j s", l=2))
             make_identity(nc, ident[:])
             nc.gpsimd.iota(pid_i[:], pattern=[[0, 1]], base=0, channel_multiplier=1)
@@ -95,36 +101,42 @@ def tile_coarsepyramid_pa_kernel(tc, feature, segments, w_lr, b_lr, g_lr, be_lr,
                                   in_=w_grp[:].rearrange("p m c j -> p (m c j)"))
         quantise_piece(0)
 
-        grp = const.tile([P, 32], F32)
-        nc.vector.tensor_reduce(out=grp[:], in_=ident[:].rearrange("p (q r) -> p q r", r=4), axis=AX.X, op=ALU.add)
-        bd = const.tile([P, 32, 4], F32)
-        nc.vector.tensor_scalar(out=bd[:], in0=grp[:].unsqueeze(2).to_broadcast([P, 32, 4]),
+        grp = const.tile([P, 16], F32)
+        nc.vector.tensor_reduce(out=grp[:], in_=ident[:].rearrange("p (q r) -> p q r", r=8), axis=AX.X, op=ALU.add)
+        bd = const.tile([P, 16, 8], F32)
+        nc.vector.tensor_scalar(out=bd[:], in0=grp[:].unsqueeze(2).to_broadcast([P, 16, 8]),
                                 scalar1=1.0 / 2048.0, scalar2=None, op0=ALU.mult)
         bd2 = bd[:].rearrange("p q r -> p (q r)")
         vec = const.tile([P, 3, NM], F32)
         for i in range(3):
             nc.vector.tensor_copy(out=vec[:, i, :], in_=vec_bf[i][:])
-        beta = vec[:, 0, :]
-        gamma = vec[:, 1, :]
-        shift0 = vec[:, 2, :]
-        beta2 = const.tile([P, NM], F32)
-        nc.vector.tensor_scalar(out=beta2[:], in0=beta, scalar1=2.0, scalar2=None, op0=ALU.mult)
+        wide = const.tile([P, 4, 2, 2, 4, 2], F32)
+        for i in range(3):
+            for e in range(2):
+                nc.vector.tensor_copy(out=wide[:, i, :, e, :, :],
+                                      in_=vec[:, i, :].rearrange("p (h i) -> p h i", h=2).unsqueeze(3).to_broadcast([P, 2, 4, 2]))
+        nc.vector.tensor_scalar(out=wide[:, 3, :, :, :, :].rearrange("p h e i l -> p (h e i l)"),
+                                in0=wide[:, 0, :, :, :, :].rearrange("p h e i l -> p (h e i l)"), scalar1=2.0, scalar2=None, op0=ALU.mult)
+        beta_w = wide[:, 0, :, :, :, :].rearrange("p h e i l -> p (h e) i l")
+        gamma_w = wide[:, 1, :, :, :, :].rearrange("p h e i l -> p (h e) i l")
+        shift_w = wide[:, 2, :, :, :, :].rearrange("p h e i l -> p (h e) i l")
+        beta2_w = wide[:, 3, :, :, :, :].rearrange("p h e i l -> p (h e) i l")
         bsq = const.tile([P, NM], F32)
-        nc.vector.tensor_tensor(out=bsq[:], in0=beta, in1=beta, op=ALU.mult)
-        cc = const.tile([P, 2], F32)
-        nc.vector.tensor_reduce(out=cc[:, 0:1], in_=beta, axis=AX.X, op=ALU.add)
-        nc.vector.tensor_reduce(out=cc[:, 1:2], in_=bsq[:], axis=AX.X, op=ALU.add)
-        cc64 = const.tile([P, 2], F32)
-        nc.vector.tensor_scalar(out=cc64[:], in0=cc[:], scalar1=64.0, scalar2=None, op0=ALU.mult)
-        cg_ps = opsum.tile([P, 2], F32, tag="op")
+        nc.vector.tensor_tensor(out=bsq[:], in0=vec[:, 0, :], in1=vec[:, 0, :], op=ALU.mult)
+        cc = const.tile([P, 2, 2], F32)
+        nc.vector.tensor_reduce(out=cc[:, 0, :], in_=vec[:, 0, :].rearrange("p (h i) -> p h i", h=2), axis=AX.X, op=ALU.add)
+        nc.vector.tensor_reduce(out=cc[:, 1, :], in_=bsq[:].rearrange("p (h i) -> p h i", h=2), axis=AX.X, op=ALU.add)
+        cc64 = const.tile([P, 4], F32)
+        nc.vector.tensor_scalar(out=cc64[:], in0=cc[:].rearrange("p s h -> p (s h)"), scalar1=64.0, scalar2=None, op0=ALU.mult)
+        cg_ps = opsum.tile([P, 4], F32, tag="op")
         nc.tensor.matmul(out=cg_ps[:], lhsT=bd2, rhs=cc64[:], start=True, stop=True)
-        cg = const.tile([P, 2], F32)
+        cg = const.tile([P, 4], F32)
         nc.vector.tensor_copy(out=cg[:], in_=cg_ps[:])
 
         idx = const.tile([P, NCH, 2, 2], I32)
 
         def gather_indices():
-            NQ = NCH * 2
+            nq = NCH * 2
             sf = const.tile([P, NCH * 4], F32)
             nc.vector.tensor_copy(out=sf[:], in_=seg_bf[:].rearrange("p j s -> p (j s)"))
             nc.vector.tensor_scalar(out=sf[:], in0=sf[:], scalar1=0.0, scalar2=float(T - 1), op0=ALU.max, op1=ALU.min)
@@ -134,106 +146,112 @@ def tile_coarsepyramid_pa_kernel(tc, feature, segments, w_lr, b_lr, g_lr, be_lr,
             nc.vector.tensor_copy(out=sr[:], in_=si[:])
             over = const.tile([P, NCH * 4], F32)
             nc.vector.tensor_tensor(out=over[:], in0=sr[:], in1=sf[:], op=ALU.is_gt)
-            fl = const.tile([P, NQ, 2], F32)
+            fl = const.tile([P, nq, 2], F32)
             nc.vector.tensor_tensor(out=fl[:].rearrange("p q e -> p (q e)"), in0=sr[:], in1=over[:], op=ALU.subtract)
             lo = fl[:, :, 0]
             hi = fl[:, :, 1]
-            ln = const.tile([P, NQ], F32)
+            ln = const.tile([P, nq], F32)
             nc.vector.tensor_tensor(out=ln[:], in0=hi, in1=lo, op=ALU.subtract)
             nc.vector.tensor_scalar(out=ln[:], in0=ln[:], scalar1=1.0, scalar2=None, op0=ALU.add)
-            valid = const.tile([P, NQ], F32)
+            valid = const.tile([P, nq], F32)
             nc.vector.tensor_scalar(out=valid[:], in0=ln[:], scalar1=1.0, scalar2=None, op0=ALU.is_ge)
-            lev256 = const.tile([P, NQ], F32)
-            wid = const.tile([P, NQ], F32)
-            nc.vector.memset(lev256[:], 0.0)
-            nc.vector.memset(wid[:], 0.0)
-            step = const.tile([P, NQ], F32)
+            lev = const.tile([P, nq], F32)
+            wid = const.tile([P, nq], F32)
+            cut = const.tile([P, nq], F32)
+            for t_ in (lev, wid, cut):
+                nc.vector.memset(t_[:], 0.0)
+            step = const.tile([P, nq], F32)
             for k in range(1, LEV):
                 nc.vector.tensor_scalar(out=step[:], in0=ln[:], scalar1=float(2 ** k), scalar2=None, op0=ALU.is_ge)
-                nc.vector.scalar_tensor_tensor(out=lev256[:], in0=step[:], scalar=256.0, in1=lev256[:], op0=ALU.mult, op1=ALU.add)
-                nc.vector.scalar_tensor_tensor(out=wid[:], in0=step[:], scalar=float(2 ** (k - 1)), in1=wid[:], op0=ALU.mult, op1=ALU.add)
+                nc.vector.scalar_tensor_tensor(out=lev[:], in0=step[:], scalar=float(2 * (ROW0[k] - ROW0[k - 1])), in1=lev[:],
+                                               op0=ALU.mult, op1=ALU.add)
+                nc.vector.scalar_tensor_tensor(out=wid[:], in0=step[:], scalar=float(2 ** (k - 1)), in1=wid[:],
+                                               op0=ALU.mult, op1=ALU.add)
+                if L_STEP[k] != L_STEP[k - 1]:
+                    nc.vector.scalar_tensor_tensor(out=cut[:], in0=step[:], scalar=float(2 * (L_STEP[k - 1] - L_STEP[k])),
+                                                   in1=cut[:], op0=ALU.mult, op1=ALU.add)
             low_i = const.tile([P, 1], I32)
-            nc.vector.tensor_single_scalar(out=low_i[:], in_=pid_i[:], scalar=15, op=ALU.bitwise_and)
+            nc.vector.tensor_single_scalar(out=low_i[:], in_=pid_i[:], scalar=3, op=ALU.bitwise_and)
             pid = const.tile([P, 1], F32)
             nc.vector.tensor_copy(out=pid[:], in_=pid_i[:])
             low = const.tile([P, 1], F32)
             nc.vector.tensor_copy(out=low[:], in_=low_i[:])
-            lbase = const.tile([P, 1], F32)
-            nc.vector.tensor_scalar(out=lbase[:], in0=pid[:], scalar1=64.0, scalar2=128.0, op0=ALU.is_ge, op1=ALU.mult)
+            l_neg = const.tile([P, 1], F32)
+            nc.vector.tensor_scalar(out=l_neg[:], in0=pid[:], scalar1=64.0, scalar2=-1.0, op0=ALU.is_ge, op1=ALU.mult)
+            z0 = const.tile([P, 1], F32)
+            nc.vector.tensor_scalar(out=z0[:], in0=low[:], scalar1=2.0, scalar2=float(2 * (ROW0[5] + 33)), op0=ALU.mult, op1=ALU.add)
             zrow = const.tile([P, 1], F32)
-            nc.vector.tensor_scalar(out=zrow[:], in0=low[:], scalar1=2.0, scalar2=float(5 * 256 + 2 * 48), op0=ALU.mult, op1=ALU.add)
-            rows = const.tile([P, NQ, 2], F32)
-            nc.vector.scalar_tensor_tensor(out=rows[:, :, 0], in0=lo, scalar=2.0, in1=lev256[:], op0=ALU.mult, op1=ALU.add)
-            t2 = const.tile([P, NQ], F32)
+            nc.vector.scalar_tensor_tensor(out=zrow[:], in0=l_neg[:], scalar=float(-2 * L_STEP[5]), in1=z0[:], op0=ALU.mult, op1=ALU.add)
+            zrel = const.tile([P, 1], F32)
+            nc.vector.scalar_tensor_tensor(out=zrel[:], in0=l_neg[:], scalar=128.0, in1=zrow[:], op0=ALU.mult, op1=ALU.add)
+            nc.vector.scalar_tensor_tensor(out=lev[:], in0=cut[:], scalar=l_neg[:, 0:1], in1=lev[:], op0=ALU.mult, op1=ALU.add)
+            rows = const.tile([P, nq, 2], F32)
+            nc.vector.scalar_tensor_tensor(out=rows[:, :, 0], in0=lo, scalar=2.0, in1=lev[:], op0=ALU.mult, op1=ALU.add)
+            t2 = const.tile([P, nq], F32)
             nc.vector.tensor_tensor(out=t2[:], in0=hi, in1=wid[:], op=ALU.subtract)
-            nc.vector.scalar_tensor_tensor(out=rows[:, :, 1], in0=t2[:], scalar=2.0, in1=lev256[:], op0=ALU.mult, op1=ALU.add)
+            nc.vector.scalar_tensor_tensor(out=rows[:, :, 1], in0=t2[:], scalar=2.0, in1=lev[:], op0=ALU.mult, op1=ALU.add)
             for e in range(2):
-                nc.vector.tensor_scalar(out=rows[:, :, e], in0=rows[:, :, e], scalar1=zrow[:, 0:1], scalar2=None, op0=ALU.subtract)
+                nc.vector.tensor_scalar(out=rows[:, :, e], in0=rows[:, :, e], scalar1=zrel[:, 0:1], scalar2=None, op0=ALU.subtract)
                 nc.vector.tensor_tensor(out=rows[:, :, e], in0=rows[:, :, e], in1=valid[:], op=ALU.mult)
-                nc.vector.tensor_scalar(out=rows[:, :, e], in0=rows[:, :, e], scalar1=zrow[:, 0:1], scalar2=lbase[:, 0:1], op0=ALU.add, op1=ALU.add)
+                nc.vector.tensor_scalar(out=rows[:, :, e], in0=rows[:, :, e], scalar1=zrow[:, 0:1], scalar2=None, op0=ALU.add)
             rows4 = rows[:].rearrange("p (j h) e -> p j h e", h=2)
             nc.vector.tensor_scalar(out=rows4[:, :, 1, :], in0=rows4[:, :, 1, :], scalar1=1.0, scalar2=None, op0=ALU.add)
             nc.vector.tensor_copy(out=idx[:].rearrange("p j h e -> p (j h e)"), in_=rows[:].rearrange("p q e -> p (q e)"))
 
-
         fpool = ctx.enter_context(tc.tile_pool(name="fpool", bufs=2))
-        late = ctx.enter_context(tc.tile_pool(name="late", bufs=6))
+        late = ctx.enter_context(tc.tile_pool(name="late", bufs=N_LATE))
         rpool = ctx.enter_context(tc.tile_pool(name="rpool", bufs=2))
-        gpool = ctx.enter_context(tc.tile_pool(name="gpool", bufs=2))
+        gpool = ctx.enter_context(tc.tile_pool(name="gpool", bufs=3))
         opool = ctx.enter_context(tc.tile_pool(name="opool", bufs=2))
 
-        slots = [out_0, out_1]
-        slot_store = [o[0:SLOT_B].rearrange("b (x c) t -> (b x) (c t)", c=16).rearrange("(k r) w -> r k w", k=LEV)
-                      for o in slots]
-        slot_rows = [o[0:SLOT_B].rearrange("b (x c) t -> (b x) (c t)", c=8) for o in slots]
+        slot_wide = [o[0:SLOT_B].rearrange("b (x c) t -> (b x) (c t)", c=16) for o in (out_0, out_1)]
+        slot_rows = [o[0:SLOT_B].rearrange("b (x c) t -> (b x) (c t)", c=8) for o in (out_0, out_1)]
 
-        def mx_passes(y, pos, hb):
+        def mx_passes(y, pos, h):
             cols = slice(P * order[pos], P * order[pos] + P)
             for i in range(4):
-                m = 4 * hb + i
+                m = 4 * h + i
                 nc.tensor.matmul_mx(out=y[:, i, :], lhsT=w_codes[:, m, :].bitcast(FP8X4), lhsT_scale=w_scales[:, m, :],
                                     rhs=x_codes[:, cols].bitcast(FP8X4), rhs_scale=x_scales[:, cols],
                                     start=True, stop=True)
 
-        def sums_mx(pos, hb):
+        def sums_mx(pos, h):
             if pos >= NCH:
                 return
-            ysum = ypsum.tile([P, 4, P], F32, name="ysum%d" % hb, tag="ysum%d" % hb)
-            mx_passes(ysum, pos, hb)
-            live[("ysum", hb)] = ysum
+            ysum = ypsum.tile([P, 4, P], F32, name="ysum%d" % h, tag="y%d" % h)
+            mx_passes(ysum, pos, h)
+            live[("ysum", h)] = ysum
 
-        def sums(pos, hb):
+        def sums(pos, h):
             if pos >= NCH:
                 return
             g, e = pos // 2, pos % 2
-            if e == 0 and hb == 0:
-                live[("s1", g)] = small.tile([P, 2, NM, 2], F32, name="s1", tag="s1")
+            if e == 0 and h == 0:
+                live[("s1", g)] = small.tile([P, 2, 2, 4, 2], F32, name="s1", tag="s1")
                 live[("acc", g)] = small.tile([P, 2, 2, 2], F32, name="acc", tag="acc")
             s1 = live[("s1", g)]
             acc = live[("acc", g)]
-            ysum = live[("ysum", hb)]
+            ysum = live[("ysum", h)]
             junk = small.tile([P, 4, T], F32)
-            nc.vector.tensor_reduce(out=s1[:, e, 4 * hb:4 * hb + 4, :].rearrange("p m l -> p (m l)"),
-                                    in_=ysum[:].rearrange("p m (l t) -> p (m l) t", l=2), axis=AX.X, op=ALU.add)
+            nc.vector.tensor_reduce(out=s1[:, h, e, :, :].rearrange("p i l -> p (i l)"),
+                                    in_=ysum[:].rearrange("p i (l t) -> p (i l) t", l=2), axis=AX.X, op=ALU.add)
             for l in range(2):
                 nc.scalar.activation(out=junk[:], in_=ysum[:, :, T * l:T * l + T], func=ACT.Square,
-                                     accum_out=acc[:, e, hb, l:l + 1])
+                                     accum_out=acc[:, h, e, l:l + 1])
 
         def chain_a(g):
             if g >= NCH // 2:
                 return
-            s1 = live[("s1", g)]
+            s1 = live[("s1", g)][:].rearrange("p h e i l -> p (h e) i l")
             acc = live[("acc", g)]
-            cross = small.tile([P, 2, NM, 2], F32)
-            nc.vector.tensor_tensor(out=cross[:], in0=s1[:],
-                                    in1=beta2[:].unsqueeze(1).unsqueeze(3).to_broadcast([P, 2, NM, 2]), op=ALU.mult)
-            rs = small.tile([P, 2, 2, 2], F32)
-            nc.vector.tensor_reduce(out=rs[:, 0, :, :], in_=s1[:].rearrange("p e m l -> p e l m"), axis=AX.X, op=ALU.add)
-            nc.vector.tensor_reduce(out=rs[:, 1, :, :], in_=cross[:].rearrange("p e m l -> p e l m"), axis=AX.X, op=ALU.add)
-            nc.vector.tensor_tensor(out=rs[:, 1, :, :], in0=rs[:, 1, :, :], in1=acc[:, :, 0, :], op=ALU.add)
-            nc.vector.tensor_tensor(out=rs[:, 1, :, :], in0=rs[:, 1, :, :], in1=acc[:, :, 1, :], op=ALU.add)
-            st = opsum.tile([P, 2, 4], F32, tag="op")
-            nc.tensor.matmul(out=st[:].rearrange("p s x -> p (s x)"), lhsT=bd2, rhs=rs[:].rearrange("p s e l -> p (s e l)"),
+            cross = small.tile([P, 4, 4, 2], F32)
+            nc.vector.tensor_tensor(out=cross[:], in0=s1, in1=beta2_w, op=ALU.mult)
+            rs = small.tile([P, 2, 4, 2], F32)
+            nc.vector.tensor_reduce(out=rs[:, 0, :, :], in_=s1.rearrange("p x i l -> p x l i"), axis=AX.X, op=ALU.add)
+            nc.vector.tensor_reduce(out=rs[:, 1, :, :], in_=cross[:].rearrange("p x i l -> p x l i"), axis=AX.X, op=ALU.add)
+            nc.vector.tensor_tensor(out=rs[:, 1, :, :], in0=rs[:, 1, :, :], in1=acc[:].rearrange("p h e l -> p (h e) l"), op=ALU.add)
+            st = opsum.tile([P, 4, 4], F32, tag="op")
+            nc.tensor.matmul(out=st[:].rearrange("p a b -> p (a b)"), lhsT=bd2, rhs=rs[:].rearrange("p s x l -> p (s x l)"),
                              start=True, stop=True)
             live[("st", g)] = st
 
@@ -241,13 +259,14 @@ def tile_coarsepyramid_pa_kernel(tc, feature, segments, w_lr, b_lr, g_lr, be_lr,
             if g >= NCH // 2:
                 return
             st = live[("st", g)]
-            mv = small.tile([P, 2, 4], F32)
-            nc.vector.tensor_tensor(out=mv[:], in0=st[:], in1=cg[:].unsqueeze(2).to_broadcast([P, 2, 4]), op=ALU.add)
-            var = small.tile([P, 4], F32)
+            mv = small.tile([P, 2, 8], F32)
+            nc.vector.tensor_tensor(out=mv[:].rearrange("p s (h x) -> p (s h) x", h=2), in0=st[:],
+                                    in1=cg[:].unsqueeze(2).to_broadcast([P, 4, 4]), op=ALU.add)
+            var = small.tile([P, 8], F32)
             nc.vector.tensor_tensor(out=var[:], in0=mv[:, 0, :], in1=mv[:, 0, :], op=ALU.mult)
             nc.vector.tensor_tensor(out=var[:], in0=mv[:, 1, :], in1=var[:], op=ALU.subtract)
             nc.vector.tensor_scalar(out=var[:], in0=var[:], scalar1=EPS, scalar2=None, op0=ALU.add)
-            std = small.tile([P, 4], F32)
+            std = small.tile([P, 8], F32)
             nc.scalar.activation(out=std[:], in_=var[:], func=ACT.Sqrt)
             live[("mv", g)] = mv
             live[("std", g)] = std
@@ -256,44 +275,45 @@ def tile_coarsepyramid_pa_kernel(tc, feature, segments, w_lr, b_lr, g_lr, be_lr,
             if g >= NCH // 2:
                 return
             mv = live[("mv", g)]
-            rstd = small.tile([P, 2, 2], F32)
-            nc.vector.reciprocal(out=rstd[:].rearrange("p e l -> p (e l)"), in_=live[("std", g)][:])
-            full = [P, 2, NM, 2]
+            rstd = small.tile([P, 4, 2], F32)
+            nc.vector.reciprocal(out=rstd[:].rearrange("p x l -> p (x l)"), in_=live[("std", g)][:])
+            full = [P, 4, 4, 2]
             sc = small.tile(full, F32)
-            nc.vector.tensor_tensor(out=sc[:], in0=gamma.unsqueeze(1).unsqueeze(3).to_broadcast(full),
-                                    in1=rstd[:].unsqueeze(2).to_broadcast(full), op=ALU.mult)
+            nc.vector.tensor_tensor(out=sc[:], in0=gamma_w, in1=rstd[:].unsqueeze(2).to_broadcast(full), op=ALU.mult)
             sh = small.tile(full, F32)
-            nc.vector.tensor_tensor(out=sh[:], in0=beta.unsqueeze(1).unsqueeze(3).to_broadcast(full),
-                                    in1=mv[:, 0, :].rearrange("p (e l) -> p e l", e=2).unsqueeze(2).to_broadcast(full),
+            nc.vector.tensor_tensor(out=sh[:], in0=beta_w,
+                                    in1=mv[:, 0, :].rearrange("p (x l) -> p x l", l=2).unsqueeze(2).to_broadcast(full),
                                     op=ALU.subtract)
             nc.vector.tensor_tensor(out=sh[:], in0=sh[:], in1=sc[:], op=ALU.mult)
-            nc.vector.tensor_tensor(out=sh[:], in0=sh[:], in1=shift0.unsqueeze(1).unsqueeze(3).to_broadcast(full), op=ALU.add)
+            nc.vector.tensor_tensor(out=sh[:], in0=sh[:], in1=shift_w, op=ALU.add)
             live[("sc", g)] = sc
             live[("sh", g)] = sh
 
         def main_mx(pos):
             ys = []
-            for hb in range(2):
-                y = ypsum.tile([P, 4, P], F32, name="y%d" % hb, tag="y%d" % hb)
-                mx_passes(y, pos, hb)
+            for h in range(2):
+                y = ypsum.tile([P, 4, P], F32, name="y%d" % h, tag="y%d" % h)
+                mx_passes(y, pos, h)
                 ys.append(y)
             live[("y", pos)] = ys
             live[("f", pos)] = fpool.tile([P, NM, P], F32, name="f", tag="f")
 
-        def apply_norm(pos, hb):
+        def apply_norm(pos, h):
             f = live[("f", pos)]
-            y = live[("y", pos)][hb]
+            y = live[("y", pos)][h]
             sc = live[("sc", pos // 2)]
             sh = live[("sh", pos // 2)]
-            e = pos % 2
+            x = 2 * h + pos % 2
             for i in range(4):
-                m = 4 * hb + i
                 for l in range(2):
-                    nc.scalar.activation(out=f[:, m, T * l:T * l + T], in_=y[:, i, T * l:T * l + T],
-                                         func=ACT.Relu, bias=sh[:, e, m, l:l + 1], scale=sc[:, e, m, l:l + 1])
+                    nc.scalar.activation(out=f[:, 4 * h + i, T * l:T * l + T], in_=y[:, i, T * l:T * l + T],
+                                         func=ACT.Relu, bias=sh[:, x, i, l:l + 1], scale=sc[:, x, i, l:l + 1])
 
-        def send(x, dst, src):
-            if held[x] is None:
+        def send(x, pos, tile_):
+            j = order[pos]
+            dst = (out_0, out_1)[x][2 * j:2 * j + 2].rearrange("l (h p i) t -> p (l h) (i t)", h=2, i=4)
+            src = tile_[:].rearrange("p l (h i) t -> p (l h) (i t)", h=2)
+            if j >= N_LATE or held[x] is None:
                 nc.sync.dma_start(out=dst, in_=src)
             else:
                 held[x].append((dst, src))
@@ -303,117 +323,107 @@ def tile_coarsepyramid_pa_kernel(tc, feature, segments, w_lr, b_lr, g_lr, be_lr,
                 nc.sync.dma_start(out=dst, in_=src)
             held[x] = None
 
+        def out_tile(pos, name):
+            if order[pos] < N_LATE:
+                return late.tile([P, 2, NM, T], F32, name=name + "_late", tag=name + "_late")
+            return opool.tile([P, 2, NM, T], F32, name=name, tag=name)
+
         def store_feat(pos):
-            j = order[pos]
-            is_late = j < SLOT_B // 2
-            f = live[("f", pos)]
-            if is_late:
-                f2 = late.tile([P, 2, NM, T], F32, name="f2_late", tag="f2_late")
-            else:
-                f2 = opool.tile([P, 2, NM, T], F32, name="f2", tag="f2")
-            nc.scalar.copy(out=f2[:], in_=f[:].rearrange("p m (l t) -> p l m t", l=2))
-            dst = out_0[2 * j:2 * j + 2].rearrange("l (p m) t -> p l (m t)", m=NM)
-            if is_late:
-                send(0, dst, f2[:].rearrange("p l m t -> p l (m t)"))
-            else:
-                nc.sync.dma_start(out=dst, in_=f2[:].rearrange("p l m t -> p l (m t)"))
+            f2 = out_tile(pos, "f2")
+            nc.scalar.copy(out=f2[:], in_=live[("f", pos)][:].rearrange("p m (l t) -> p l m t", l=2))
+            send(0, pos, f2)
+
+        def level(pos, k):
+            if k == 0:
+                return live[("f", pos)][:].rearrange("p m (l t) -> p m l t", l=2)
+            return tab[:, k - 1, :, 0:2 * L_STEP[k]].rearrange("p m (l t) -> p m l t", l=2)
 
         def level_up(pos, k):
             s = 2 ** k
             n_ok = T - 2 * s + 1
-            if k == 0:
-                prev = live[("f", pos)][:].rearrange("p m (l t) -> p (m l) t", l=2)
-            else:
-                prev = tab[:, k - 1, :, :].rearrange("p m (l t) -> p (m l) t", l=2)
-            nxt = tab[:, k, :, :].rearrange("p m (l t) -> p (m l) t", l=2)
-            nc.vector.tensor_tensor(out=nxt[:, :, 0:n_ok], in0=prev[:, :, 0:n_ok], in1=prev[:, :, s:s + n_ok], op=ALU.max)
+            prev = level(pos, k)
+            nc.vector.tensor_tensor(out=level(pos, k + 1)[:, :, :, 0:n_ok], in0=prev[:, :, :, 0:n_ok],
+                                    in1=prev[:, :, :, s:s + n_ok], op=ALU.max)
 
         def rows_out(pos, k):
-            f = live[("f", pos)]
             if k == 0:
-                live[("r", pos)] = rpool.tile([P, LEV, 2, NM, 64], F32, name="r", tag="r")
+                live[("r", pos)] = rpool.tile([P, LEV, 2, C], F32, name="r", tag="r")
             r = live[("r", pos)]
-            for hb in range(2):
+            for h in range(2):
                 tp = tpsum.tile([P, 4, P], F32, tag="tp")
                 for i in range(4):
-                    m = 4 * hb + i
-                    src = f[:, m, :] if k == 0 else tab[:, k - 1, m, :]
+                    m = 4 * h + i
+                    src = live[("f", pos)][:, m, :] if k == 0 else tab[:, k - 1, m, :]
                     nc.tensor.transpose(tp[:, i, :], src, ident[:])
-                dst = r[:, k, :, 4 * hb:4 * hb + 4, :]
-                view = tp[:].rearrange("p m (h q) -> p h m q", h=2)
                 if k >= 4:
-                    nc.vector.tensor_copy(out=dst, in_=view)
+                    nc.vector.tensor_copy(out=r[:, k, h, :], in_=tp[:].rearrange("p i q -> p (i q)"))
                 else:
-                    nc.scalar.copy(out=dst, in_=view)
-            if k % 2 == 1:
-                nc.sync.dma_start(out=slot_store[pos % 2][:, k - 1:k + 1, :],
-                                  in_=r[:, k - 1:k + 1, :, :, :].rearrange("p k h m q -> p k (h m q)"))
+                    nc.scalar.copy(out=r[:, k, h, :], in_=tp[:].rearrange("p i q -> p (i q)"))
+            slot = slot_wide[pos % 2]
+            if k in (1, 3):
+                nc.sync.dma_start(out=slot[ROW0[k - 1]:ROW0[k - 1] + 2 * P, :].rearrange("(k r) w -> r k w", k=2),
+                                  in_=r[:, k - 1:k + 1, :, :].rearrange("p k h c -> p k (h c)"))
+            if k >= 4:
+                n_r = 2 * L_STEP[k]
+                nc.sync.dma_start(out=slot[ROW0[k]:ROW0[k] + n_r, :], in_=r[0:n_r, k, :, :].rearrange("p h c -> p (h c)"))
 
         def gathers(pos):
             j = order[pos]
             got = []
             for h in range(2):
-                ga = gpool.tile([P, C], F32, name="ga%d" % h, tag="ga%d" % h, bufs=3)
-                gb = gpool.tile([P, C], F32, name="gb%d" % h, tag="gb%d" % h, bufs=3)
-                nc.gpsimd.indirect_dma_start(out=ga[:], out_offset=None, in_=slot_rows[pos % 2],
-                                             in_offset=bass.IndirectOffsetOnAxis(ap=idx[:, j, h, 0:1], axis=0))
-                nc.gpsimd.indirect_dma_start(out=gb[:], out_offset=None, in_=slot_rows[pos % 2],
-                                             in_offset=bass.IndirectOffsetOnAxis(ap=idx[:, j, h, 1:2], axis=0))
-                got.append((ga, gb))
+                pair = []
+                for e in range(2):
+                    ga = gpool.tile([P, C], F32, name="g%d%d" % (h, e), tag="g%d%d" % (h, e))
+                    nc.gpsimd.indirect_dma_start(out=ga[:], out_offset=None, in_=slot_rows[pos % 2],
+                                                 in_offset=bass.IndirectOffsetOnAxis(ap=idx[:, j, h, e:e + 1], axis=0))
+                    pair.append(ga)
+                got.append(pair)
             live[("g", pos)] = got
 
-        def window_max(pos):
-            gc = gpool.tile([P, NM, 2, 64], F32)
-            for h in range(2):
-                ga, gb = live[("g", pos)][h]
-                nc.vector.tensor_tensor(out=gc[:, :, h, :], in0=ga[:].rearrange("p (m q) -> p m q", m=NM),
-                                        in1=gb[:].rearrange("p (m q) -> p m q", m=NM), op=ALU.max)
-            live[("gc", pos)] = gc
+        def pooled_turn(pos, h):
+            banks = []
+            for e in range(2):
+                bank = opsum.tile([P, 4, P], F32, name="bank", tag="op")
+                for i in range(4):
+                    nc.tensor.transpose(bank[:, i, :], live[("g", pos)][h][e][:, P * i:P * i + P], ident[:])
+                banks.append(bank)
+                if e == 0:
+                    one = opool.tile([P, 4, P], F32, name="one", tag="one")
+                    nc.scalar.copy(out=one[:], in_=bank[:])
+            live[("turn", pos, h)] = (one, banks[1])
 
-        def pooled_out(pos, hb):
-            j = order[pos]
-            is_late = j < SLOT_B // 2
-            gc = live[("gc", pos)]
-            if hb == 0:
-                if is_late:
-                    live[("o", pos)] = late.tile([P, 2, NM, T], F32, name="o_late", tag="o_late")
-                else:
-                    live[("o", pos)] = opool.tile([P, 2, NM, T], F32, name="o", tag="o")
+        def pooled_max(pos, h):
+            if h == 0:
+                live[("o", pos)] = out_tile(pos, "o")
             o = live[("o", pos)]
-            op = opsum.tile([P, 4, P], F32, tag="op")
-            for i in range(4):
-                nc.tensor.transpose(op[:, i, :], gc[:, 4 * hb + i, :, :].rearrange("p h q -> p (h q)"), ident[:])
-            nc.scalar.copy(out=o[:, :, 4 * hb:4 * hb + 4, :], in_=op[:].rearrange("p m (l n) -> p l m n", l=2))
-            if hb == 1:
-                dst = out_1[2 * j:2 * j + 2].rearrange("l (p m) n -> p l (m n)", m=NM)
-                if is_late:
-                    send(1, dst, o[:].rearrange("p l m n -> p l (m n)"))
-                else:
-                    nc.sync.dma_start(out=dst, in_=o[:].rearrange("p l m n -> p l (m n)"))
+            one, bank = live[("turn", pos, h)]
+            nc.vector.tensor_tensor(out=o[:, :, 4 * h:4 * h + 4, :], in0=bank[:].rearrange("p i (l n) -> p l i n", l=2),
+                                    in1=one[:].rearrange("p i (l n) -> p l i n", l=2), op=ALU.max)
+            if h == 1:
+                send(1, pos, o)
 
         for pos in range(2):
-            for hb in range(2):
-                sums_mx(pos, hb)
-                sums(pos, hb)
+            for h in range(2):
+                sums_mx(pos, h)
+                sums(pos, h)
         chain_a(0)
         chain_b(0)
         chain_c(0)
-        for a in range(NCH + 4):
+        for a in range(NCH + 3):
             first = a < NCH
             second = 0 <= a - 1 < NCH
             third = 0 <= a - 3 < NCH
-            fourth = 0 <= a - 4 < NCH
             g_next = (a + 1) // 2 if a % 2 == 1 else NCH
             for q in range(2, len(pieces)):
                 if first_use(q) - 6 == a:
                     load_piece(q)
-            if fourth:
-                pooled_out(a - 4, 0)
             if second:
                 rows_out(a - 1, 0)
                 level_up(a - 1, 0)
             if first:
                 main_mx(a)
+            if third:
+                pooled_turn(a - 3, 0)
             if second:
                 level_up(a - 1, 1)
                 rows_out(a - 1, 1)
@@ -422,34 +432,36 @@ def tile_coarsepyramid_pa_kernel(tc, feature, segments, w_lr, b_lr, g_lr, be_lr,
                 apply_norm(a, 1)
                 store_feat(a)
                 quantise_piece(1)
-                for hb in range(2):
-                    sums_mx(2, hb)
-                    sums(2, hb)
+                for h in range(2):
+                    sums_mx(2, h)
+                    sums(2, h)
                 gather_indices()
-            sums_mx(a + 3, 0)
-            sums_mx(a + 3, 1)
             if second:
                 level_up(a - 1, 2)
                 rows_out(a - 1, 2)
                 level_up(a - 1, 3)
+            if third:
+                pooled_turn(a - 3, 1)
+            if second:
                 rows_out(a - 1, 3)
                 level_up(a - 1, 4)
                 rows_out(a - 1, 4)
                 rows_out(a - 1, 5)
                 gathers(a - 1)
+            if third:
+                pooled_max(a - 3, 0)
+                pooled_max(a - 3, 1)
+                if a - 3 >= NCH - 2:
+                    give_up_slot((a - 3) % 2)
             chain_a(g_next)
             if first and a > 0:
                 apply_norm(a, 0)
                 apply_norm(a, 1)
                 store_feat(a)
+            sums_mx(a + 3, 0)
+            sums_mx(a + 3, 1)
             sums(a + 3, 0)
             chain_b(g_next)
-            if third:
-                window_max(a - 3)
-                if a - 3 >= NCH - 2:
-                    give_up_slot((a - 3) % 2)
-            if fourth:
-                pooled_out(a - 4, 1)
             sums(a + 3, 1)
             chain_c(g_next)
             for q in range(2, len(pieces)):

@@ -20,11 +20,7 @@ NM = 8
 NCH = B // 2
 LEV = 6
 EPS = 1e-5
-L_STEP = [64, 64, 64, 64, 56, 40]
-ROW0 = [0, 128, 256, 384, 512, 624]
-N_ROWS = 704
-SLOT_B = 11
-N_LATE = 6
+SLOT_B = 12
 FLOPS = 2 * B * C2 * C * T
 
 
@@ -35,10 +31,10 @@ def tile_coarsepyramid_pa_kernel(tc, feature, segments, w_lr, b_lr, g_lr, be_lr,
         small = ctx.enter_context(tc.tile_pool(name="small", bufs=3))
         stage = ctx.enter_context(tc.tile_pool(name="stage", bufs=2))
         ypsum = ctx.enter_context(tc.psum_pool(name="ypsum", bufs=1))
-        tpsum = ctx.enter_context(tc.psum_pool(name="tpsum", bufs=4))
-        opsum = ctx.enter_context(tc.psum_pool(name="opsum", bufs=2))
+        tpsum = ctx.enter_context(tc.psum_pool(name="tpsum", bufs=3))
+        opsum = ctx.enter_context(tc.psum_pool(name="opsum", bufs=1))
 
-        order = list(range(N_LATE, NCH)) + list(range(N_LATE))
+        order = list(range(SLOT_B // 2, NCH)) + list(range(SLOT_B // 2))
         live = {}
         held = {0: [], 1: []}
 
@@ -74,13 +70,11 @@ def tile_coarsepyramid_pa_kernel(tc, feature, segments, w_lr, b_lr, g_lr, be_lr,
         pid_i = const.tile([P, 1], I32)
         with tc.tile_pool(name="wstage", bufs=1) as wstage:
             w_sb = wstage.tile([P, NM, C], BF16)
-            nc.sync.dma_start(out=w_sb[:].rearrange("p (h i) k -> p h (i k)", h=2),
-                              in_=w_lr.rearrange("(h p i) k -> p h (i k)", h=2, i=4))
+            nc.sync.dma_start(out=w_sb[:], in_=w_lr.rearrange("(p m) k -> p m k", m=NM))
             load_piece(0)
             load_piece(1)
             for i, v in enumerate((b_lr, g_lr, be_lr)):
-                nc.scalar.dma_start(out=vec_bf[i][:].rearrange("p (h i) -> p h i", h=2),
-                                    in_=v.rearrange("(h p i) -> p h i", h=2, i=4))
+                nc.scalar.dma_start(out=vec_bf[i][:], in_=v.rearrange("(p m) -> p m", m=NM))
             nc.scalar.dma_start(out=seg_bf[:], in_=segments.rearrange("(j l) n s -> (l n) j s", l=2))
             make_identity(nc, ident[:])
             nc.gpsimd.iota(pid_i[:], pattern=[[0, 1]], base=0, channel_multiplier=1)
@@ -101,42 +95,36 @@ def tile_coarsepyramid_pa_kernel(tc, feature, segments, w_lr, b_lr, g_lr, be_lr,
                                   in_=w_grp[:].rearrange("p m c j -> p (m c j)"))
         quantise_piece(0)
 
-        grp = const.tile([P, 16], F32)
-        nc.vector.tensor_reduce(out=grp[:], in_=ident[:].rearrange("p (q r) -> p q r", r=8), axis=AX.X, op=ALU.add)
-        bd = const.tile([P, 16, 8], F32)
-        nc.vector.tensor_scalar(out=bd[:], in0=grp[:].unsqueeze(2).to_broadcast([P, 16, 8]),
+        grp = const.tile([P, 32], F32)
+        nc.vector.tensor_reduce(out=grp[:], in_=ident[:].rearrange("p (q r) -> p q r", r=4), axis=AX.X, op=ALU.add)
+        bd = const.tile([P, 32, 4], F32)
+        nc.vector.tensor_scalar(out=bd[:], in0=grp[:].unsqueeze(2).to_broadcast([P, 32, 4]),
                                 scalar1=1.0 / 2048.0, scalar2=None, op0=ALU.mult)
         bd2 = bd[:].rearrange("p q r -> p (q r)")
         vec = const.tile([P, 3, NM], F32)
         for i in range(3):
             nc.vector.tensor_copy(out=vec[:, i, :], in_=vec_bf[i][:])
-        wide = const.tile([P, 4, 2, 2, 4, 2], F32)
-        for i in range(3):
-            for e in range(2):
-                nc.vector.tensor_copy(out=wide[:, i, :, e, :, :],
-                                      in_=vec[:, i, :].rearrange("p (h i) -> p h i", h=2).unsqueeze(3).to_broadcast([P, 2, 4, 2]))
-        nc.vector.tensor_scalar(out=wide[:, 3, :, :, :, :].rearrange("p h e i l -> p (h e i l)"),
-                                in0=wide[:, 0, :, :, :, :].rearrange("p h e i l -> p (h e i l)"), scalar1=2.0, scalar2=None, op0=ALU.mult)
-        beta_w = wide[:, 0, :, :, :, :].rearrange("p h e i l -> p (h e) i l")
-        gamma_w = wide[:, 1, :, :, :, :].rearrange("p h e i l -> p (h e) i l")
-        shift_w = wide[:, 2, :, :, :, :].rearrange("p h e i l -> p (h e) i l")
-        beta2_w = wide[:, 3, :, :, :, :].rearrange("p h e i l -> p (h e) i l")
+        beta = vec[:, 0, :]
+        gamma = vec[:, 1, :]
+        shift0 = vec[:, 2, :]
+        beta2 = const.tile([P, NM], F32)
+        nc.vector.tensor_scalar(out=beta2[:], in0=beta, scalar1=2.0, scalar2=None, op0=ALU.mult)
         bsq = const.tile([P, NM], F32)
-        nc.vector.tensor_tensor(out=bsq[:], in0=vec[:, 0, :], in1=vec[:, 0, :], op=ALU.mult)
-        cc = const.tile([P, 2, 2], F32)
-        nc.vector.tensor_reduce(out=cc[:, 0, :], in_=vec[:, 0, :].rearrange("p (h i) -> p h i", h=2), axis=AX.X, op=ALU.add)
-        nc.vector.tensor_reduce(out=cc[:, 1, :], in_=bsq[:].rearrange("p (h i) -> p h i", h=2), axis=AX.X, op=ALU.add)
-        cc64 = const.tile([P, 4], F32)
-        nc.vector.tensor_scalar(out=cc64[:], in0=cc[:].rearrange("p s h -> p (s h)"), scalar1=64.0, scalar2=None, op0=ALU.mult)
-        cg_ps = opsum.tile([P, 4], F32, tag="op")
+        nc.vector.tensor_tensor(out=bsq[:], in0=beta, in1=beta, op=ALU.mult)
+        cc = const.tile([P, 2], F32)
+        nc.vector.tensor_reduce(out=cc[:, 0:1], in_=beta, axis=AX.X, op=ALU.add)
+        nc.vector.tensor_reduce(out=cc[:, 1:2], in_=bsq[:], axis=AX.X, op=ALU.add)
+        cc64 = const.tile([P, 2], F32)
+        nc.vector.tensor_scalar(out=cc64[:], in0=cc[:], scalar1=64.0, scalar2=None, op0=ALU.mult)
+        cg_ps = opsum.tile([P, 2], F32, tag="op")
         nc.tensor.matmul(out=cg_ps[:], lhsT=bd2, rhs=cc64[:], start=True, stop=True)
-        cg = const.tile([P, 4], F32)
+        cg = const.tile([P, 2], F32)
         nc.vector.tensor_copy(out=cg[:], in_=cg_ps[:])
 
         idx = const.tile([P, NCH, 2, 2], I32)
 
         def gather_indices():
-            nq = NCH * 2
+            NQ = NCH * 2
             sf = const.tile([P, NCH * 4], F32)
             nc.vector.tensor_copy(out=sf[:], in_=seg_bf[:].rearrange("p j s -> p (j s)"))
             nc.vector.tensor_scalar(out=sf[:], in0=sf[:], scalar1=0.0, scalar2=float(T - 1), op0=ALU.max, op1=ALU.min)
@@ -146,112 +134,106 @@ def tile_coarsepyramid_pa_kernel(tc, feature, segments, w_lr, b_lr, g_lr, be_lr,
             nc.vector.tensor_copy(out=sr[:], in_=si[:])
             over = const.tile([P, NCH * 4], F32)
             nc.vector.tensor_tensor(out=over[:], in0=sr[:], in1=sf[:], op=ALU.is_gt)
-            fl = const.tile([P, nq, 2], F32)
+            fl = const.tile([P, NQ, 2], F32)
             nc.vector.tensor_tensor(out=fl[:].rearrange("p q e -> p (q e)"), in0=sr[:], in1=over[:], op=ALU.subtract)
             lo = fl[:, :, 0]
             hi = fl[:, :, 1]
-            ln = const.tile([P, nq], F32)
+            ln = const.tile([P, NQ], F32)
             nc.vector.tensor_tensor(out=ln[:], in0=hi, in1=lo, op=ALU.subtract)
             nc.vector.tensor_scalar(out=ln[:], in0=ln[:], scalar1=1.0, scalar2=None, op0=ALU.add)
-            valid = const.tile([P, nq], F32)
+            valid = const.tile([P, NQ], F32)
             nc.vector.tensor_scalar(out=valid[:], in0=ln[:], scalar1=1.0, scalar2=None, op0=ALU.is_ge)
-            lev = const.tile([P, nq], F32)
-            wid = const.tile([P, nq], F32)
-            cut = const.tile([P, nq], F32)
-            for t_ in (lev, wid, cut):
-                nc.vector.memset(t_[:], 0.0)
-            step = const.tile([P, nq], F32)
+            lev256 = const.tile([P, NQ], F32)
+            wid = const.tile([P, NQ], F32)
+            nc.vector.memset(lev256[:], 0.0)
+            nc.vector.memset(wid[:], 0.0)
+            step = const.tile([P, NQ], F32)
             for k in range(1, LEV):
                 nc.vector.tensor_scalar(out=step[:], in0=ln[:], scalar1=float(2 ** k), scalar2=None, op0=ALU.is_ge)
-                nc.vector.scalar_tensor_tensor(out=lev[:], in0=step[:], scalar=float(2 * (ROW0[k] - ROW0[k - 1])), in1=lev[:],
-                                               op0=ALU.mult, op1=ALU.add)
-                nc.vector.scalar_tensor_tensor(out=wid[:], in0=step[:], scalar=float(2 ** (k - 1)), in1=wid[:],
-                                               op0=ALU.mult, op1=ALU.add)
-                if L_STEP[k] != L_STEP[k - 1]:
-                    nc.vector.scalar_tensor_tensor(out=cut[:], in0=step[:], scalar=float(2 * (L_STEP[k - 1] - L_STEP[k])),
-                                                   in1=cut[:], op0=ALU.mult, op1=ALU.add)
+                nc.vector.scalar_tensor_tensor(out=lev256[:], in0=step[:], scalar=2.0, in1=lev256[:], op0=ALU.mult, op1=ALU.add)
+                nc.vector.scalar_tensor_tensor(out=wid[:], in0=step[:], scalar=float(2 ** (k - 1)), in1=wid[:], op0=ALU.mult, op1=ALU.add)
             low_i = const.tile([P, 1], I32)
-            nc.vector.tensor_single_scalar(out=low_i[:], in_=pid_i[:], scalar=3, op=ALU.bitwise_and)
+            nc.vector.tensor_single_scalar(out=low_i[:], in_=pid_i[:], scalar=15, op=ALU.bitwise_and)
             pid = const.tile([P, 1], F32)
             nc.vector.tensor_copy(out=pid[:], in_=pid_i[:])
             low = const.tile([P, 1], F32)
             nc.vector.tensor_copy(out=low[:], in_=low_i[:])
-            l_neg = const.tile([P, 1], F32)
-            nc.vector.tensor_scalar(out=l_neg[:], in0=pid[:], scalar1=64.0, scalar2=-1.0, op0=ALU.is_ge, op1=ALU.mult)
-            z0 = const.tile([P, 1], F32)
-            nc.vector.tensor_scalar(out=z0[:], in0=low[:], scalar1=2.0, scalar2=float(2 * (ROW0[5] + 33)), op0=ALU.mult, op1=ALU.add)
+            lbase = const.tile([P, 1], F32)
+            nc.vector.tensor_scalar(out=lbase[:], in0=pid[:], scalar1=64.0, scalar2=768.0, op0=ALU.is_ge, op1=ALU.mult)
             zrow = const.tile([P, 1], F32)
-            nc.vector.scalar_tensor_tensor(out=zrow[:], in0=l_neg[:], scalar=float(-2 * L_STEP[5]), in1=z0[:], op0=ALU.mult, op1=ALU.add)
-            zrel = const.tile([P, 1], F32)
-            nc.vector.scalar_tensor_tensor(out=zrel[:], in0=l_neg[:], scalar=128.0, in1=zrow[:], op0=ALU.mult, op1=ALU.add)
-            nc.vector.scalar_tensor_tensor(out=lev[:], in0=cut[:], scalar=l_neg[:, 0:1], in1=lev[:], op0=ALU.mult, op1=ALU.add)
-            rows = const.tile([P, nq, 2], F32)
-            nc.vector.scalar_tensor_tensor(out=rows[:, :, 0], in0=lo, scalar=2.0, in1=lev[:], op0=ALU.mult, op1=ALU.add)
-            t2 = const.tile([P, nq], F32)
+            nc.vector.tensor_scalar(out=zrow[:], in0=low[:], scalar1=12.0, scalar2=float(12 * 48 + 2 * 5), op0=ALU.mult, op1=ALU.add)
+            rows = const.tile([P, NQ, 2], F32)
+            nc.vector.scalar_tensor_tensor(out=rows[:, :, 0], in0=lo, scalar=12.0, in1=lev256[:], op0=ALU.mult, op1=ALU.add)
+            t2 = const.tile([P, NQ], F32)
             nc.vector.tensor_tensor(out=t2[:], in0=hi, in1=wid[:], op=ALU.subtract)
-            nc.vector.scalar_tensor_tensor(out=rows[:, :, 1], in0=t2[:], scalar=2.0, in1=lev[:], op0=ALU.mult, op1=ALU.add)
+            nc.vector.scalar_tensor_tensor(out=rows[:, :, 1], in0=t2[:], scalar=12.0, in1=lev256[:], op0=ALU.mult, op1=ALU.add)
             for e in range(2):
-                nc.vector.tensor_scalar(out=rows[:, :, e], in0=rows[:, :, e], scalar1=zrel[:, 0:1], scalar2=None, op0=ALU.subtract)
+                nc.vector.tensor_scalar(out=rows[:, :, e], in0=rows[:, :, e], scalar1=zrow[:, 0:1], scalar2=None, op0=ALU.subtract)
                 nc.vector.tensor_tensor(out=rows[:, :, e], in0=rows[:, :, e], in1=valid[:], op=ALU.mult)
-                nc.vector.tensor_scalar(out=rows[:, :, e], in0=rows[:, :, e], scalar1=zrow[:, 0:1], scalar2=None, op0=ALU.add)
+                nc.vector.tensor_scalar(out=rows[:, :, e], in0=rows[:, :, e], scalar1=zrow[:, 0:1], scalar2=lbase[:, 0:1], op0=ALU.add, op1=ALU.add)
             rows4 = rows[:].rearrange("p (j h) e -> p j h e", h=2)
             nc.vector.tensor_scalar(out=rows4[:, :, 1, :], in0=rows4[:, :, 1, :], scalar1=1.0, scalar2=None, op0=ALU.add)
             nc.vector.tensor_copy(out=idx[:].rearrange("p j h e -> p (j h e)"), in_=rows[:].rearrange("p q e -> p (q e)"))
 
+
         fpool = ctx.enter_context(tc.tile_pool(name="fpool", bufs=2))
-        late = ctx.enter_context(tc.tile_pool(name="late", bufs=N_LATE))
+        late = ctx.enter_context(tc.tile_pool(name="late", bufs=6))
         rpool = ctx.enter_context(tc.tile_pool(name="rpool", bufs=2))
-        gpool = ctx.enter_context(tc.tile_pool(name="gpool", bufs=3))
+        gpool = ctx.enter_context(tc.tile_pool(name="gpool", bufs=2))
         opool = ctx.enter_context(tc.tile_pool(name="opool", bufs=2))
 
-        slot_wide = [o[0:SLOT_B].rearrange("b (x c) t -> (b x) (c t)", c=16) for o in (out_0, out_1)]
-        slot_rows = [o[0:SLOT_B].rearrange("b (x c) t -> (b x) (c t)", c=8) for o in (out_0, out_1)]
+        slots = [out_0, out_1]
+        slot_store = [o[0:SLOT_B].rearrange("b (x c) t -> (b x) (c t)", c=16).rearrange("(r k) w -> r k w", k=LEV)
+                      for o in slots]
+        slot_rows = [o[0:SLOT_B].rearrange("b (x c) t -> (b x) (c t)", c=8) for o in slots]
 
-        def mx_passes(y, pos, h):
+        def mx_passes(y, pos, hb):
             cols = slice(P * order[pos], P * order[pos] + P)
             for i in range(4):
-                m = 4 * h + i
+                m = 4 * hb + i
                 nc.tensor.matmul_mx(out=y[:, i, :], lhsT=w_codes[:, m, :].bitcast(FP8X4), lhsT_scale=w_scales[:, m, :],
                                     rhs=x_codes[:, cols].bitcast(FP8X4), rhs_scale=x_scales[:, cols],
                                     start=True, stop=True)
 
-        def sums_mx(pos, h):
+        def sums_mx(pos, hb):
             if pos >= NCH:
                 return
-            ysum = ypsum.tile([P, 4, P], F32, name="ysum%d" % h, tag="y%d" % h)
-            mx_passes(ysum, pos, h)
-            live[("ysum", h)] = ysum
+            ysum = ypsum.tile([P, 4, P], F32, name="ysum%d" % hb, tag="ysum%d" % hb)
+            mx_passes(ysum, pos, hb)
+            live[("ysum", hb)] = ysum
 
-        def sums(pos, h):
+        def sums(pos, hb):
             if pos >= NCH:
                 return
             g, e = pos // 2, pos % 2
-            if e == 0 and h == 0:
-                live[("s1", g)] = small.tile([P, 2, 2, 4, 2], F32, name="s1", tag="s1")
+            if e == 0 and hb == 0:
+                live[("s1", g)] = small.tile([P, 2, NM, 2], F32, name="s1", tag="s1")
                 live[("acc", g)] = small.tile([P, 2, 2, 2], F32, name="acc", tag="acc")
             s1 = live[("s1", g)]
             acc = live[("acc", g)]
-            ysum = live[("ysum", h)]
+            ysum = live[("ysum", hb)]
             junk = small.tile([P, 4, T], F32)
-            nc.vector.tensor_reduce(out=s1[:, h, e, :, :].rearrange("p i l -> p (i l)"),
-                                    in_=ysum[:].rearrange("p i (l t) -> p (i l) t", l=2), axis=AX.X, op=ALU.add)
+            nc.vector.tensor_reduce(out=s1[:, e, 4 * hb:4 * hb + 4, :].rearrange("p m l -> p (m l)"),
+                                    in_=ysum[:].rearrange("p m (l t) -> p (m l) t", l=2), axis=AX.X, op=ALU.add)
             for l in range(2):
                 nc.scalar.activation(out=junk[:], in_=ysum[:, :, T * l:T * l + T], func=ACT.Square,
-                                     accum_out=acc[:, h, e, l:l + 1])
+                                     accum_out=acc[:, e, hb, l:l + 1])
 
         def chain_a(g):
             if g >= NCH // 2:
                 return
-            s1 = live[("s1", g)][:].rearrange("p h e i l -> p (h e) i l")
+            s1 = live[("s1", g)]
             acc = live[("acc", g)]
-            cross = small.tile([P, 4, 4, 2], F32)
-            nc.vector.tensor_tensor(out=cross[:], in0=s1, in1=beta2_w, op=ALU.mult)
-            rs = small.tile([P, 2, 4, 2], F32)
-            nc.vector.tensor_reduce(out=rs[:, 0, :, :], in_=s1.rearrange("p x i l -> p x l i"), axis=AX.X, op=ALU.add)
-            nc.vector.tensor_reduce(out=rs[:, 1, :, :], in_=cross[:].rearrange("p x i l -> p x l i"), axis=AX.X, op=ALU.add)
-            nc.vector.tensor_tensor(out=rs[:, 1, :, :], in0=rs[:, 1, :, :], in1=acc[:].rearrange("p h e l -> p (h e) l"), op=ALU.add)
-            st = opsum.tile([P, 4, 4], F32, tag="op")
-            nc.tensor.matmul(out=st[:].rearrange("p a b -> p (a b)"), lhsT=bd2, rhs=rs[:].rearrange("p s x l -> p (s x l)"),
+            cross = small.tile([P, 2, NM, 2], F32)
+            nc.vector.tensor_tensor(out=cross[:], in0=s1[:],
+                                    in1=beta2[:].unsqueeze(1).unsqueeze(3).to_broadcast([P, 2, NM, 2]), op=ALU.mult)
+            rs = small.tile([P, 2, 2, 2], F32)
+            nc.vector.tensor_reduce(out=rs[:, 0, :, :], in_=s1[:].rearrange("p e m l -> p e l m"), axis=AX.X, op=ALU.add)
+            nc.vector.tensor_reduce(out=rs[:, 1, :, :], in_=cross[:].rearrange("p e m l -> p e l m"), axis=AX.X, op=ALU.add)
+            nc.vector.tensor_tensor(out=rs[:, 1, :, :], in0=rs[:, 1, :, :], in1=acc[:, :, 0, :], op=ALU.add)
+            nc.vector.tensor_tensor(out=rs[:, 1, :, :], in0=rs[:, 1, :, :], in1=acc[:, :, 1, :], op=ALU.add)
+            st = opsum.tile([P, 2, 4], F32, tag="op")
+            nc.tensor.matmul(out=st[:].rearrange("p s x -> p (s x)"), lhsT=bd2, rhs=rs[:].rearrange("p s e l -> p (s e l)"),
                              start=True, stop=True)
             live[("st", g)] = st
 
@@ -259,14 +241,13 @@ def tile_coarsepyramid_pa_kernel(tc, feature, segments, w_lr, b_lr, g_lr, be_lr,
             if g >= NCH // 2:
                 return
             st = live[("st", g)]
-            mv = small.tile([P, 2, 8], F32)
-            nc.vector.tensor_tensor(out=mv[:].rearrange("p s (h x) -> p (s h) x", h=2), in0=st[:],
-                                    in1=cg[:].unsqueeze(2).to_broadcast([P, 4, 4]), op=ALU.add)
-            var = small.tile([P, 8], F32)
+            mv = small.tile([P, 2, 4], F32)
+            nc.vector.tensor_tensor(out=mv[:], in0=st[:], in1=cg[:].unsqueeze(2).to_broadcast([P, 2, 4]), op=ALU.add)
+            var = small.tile([P, 4], F32)
             nc.vector.tensor_tensor(out=var[:], in0=mv[:, 0, :], in1=mv[:, 0, :], op=ALU.mult)
             nc.vector.tensor_tensor(out=var[:], in0=mv[:, 1, :], in1=var[:], op=ALU.subtract)
             nc.vector.tensor_scalar(out=var[:], in0=var[:], scalar1=EPS, scalar2=None, op0=ALU.add)
-            std = small.tile([P, 8], F32)
+            std = small.tile([P, 4], F32)
             nc.scalar.activation(out=std[:], in_=var[:], func=ACT.Sqrt)
             live[("mv", g)] = mv
             live[("std", g)] = std
@@ -275,45 +256,44 @@ def tile_coarsepyramid_pa_kernel(tc, feature, segments, w_lr, b_lr, g_lr, be_lr,
             if g >= NCH // 2:
                 return
             mv = live[("mv", g)]
-            rstd = small.tile([P, 4, 2], F32)
-            nc.vector.reciprocal(out=rstd[:].rearrange("p x l -> p (x l)"), in_=live[("std", g)][:])
-            full = [P, 4, 4, 2]
+            rstd = small.tile([P, 2, 2], F32)
+            nc.vector.reciprocal(out=rstd[:].rearrange("p e l -> p (e l)"), in_=live[("std", g)][:])
+            full = [P, 2, NM, 2]
             sc = small.tile(full, F32)
-            nc.vector.tensor_tensor(out=sc[:], in0=gamma_w, in1=rstd[:].unsqueeze(2).to_broadcast(full), op=ALU.mult)
+            nc.vector.tensor_tensor(out=sc[:], in0=gamma.unsqueeze(1).unsqueeze(3).to_broadcast(full),
+                                    in1=rstd[:].unsqueeze(2).to_broadcast(full), op=ALU.mult)
             sh = small.tile(full, F32)
-            nc.vector.tensor_tensor(out=sh[:], in0=beta_w,
-                                    in1=mv[:, 0, :].rearrange("p (x l) -> p x l", l=2).unsqueeze(2).to_broadcast(full),
+            nc.vector.tensor_tensor(out=sh[:], in0=beta.unsqueeze(1).unsqueeze(3).to_broadcast(full),
+                                    in1=mv[:, 0, :].rearrange("p (e l) -> p e l", e=2).unsqueeze(2).to_broadcast(full),
                                     op=ALU.subtract)
             nc.vector.tensor_tensor(out=sh[:], in0=sh[:], in1=sc[:], op=ALU.mult)
-            nc.vector.tensor_tensor(out=sh[:], in0=sh[:], in1=shift_w, op=ALU.add)
+            nc.vector.tensor_tensor(out=sh[:], in0=sh[:], in1=shift0.unsqueeze(1).unsqueeze(3).to_broadcast(full), op=ALU.add)
             live[("sc", g)] = sc
             live[("sh", g)] = sh
 
         def main_mx(pos):
             ys = []
-            for h in range(2):
-                y = ypsum.tile([P, 4, P], F32, name="y%d" % h, tag="y%d" % h)
-                mx_passes(y, pos, h)
+            for hb in range(2):
+                y = ypsum.tile([P, 4, P], F32, name="y%d" % hb, tag="y%d" % hb)
+                mx_passes(y, pos, hb)
                 ys.append(y)
             live[("y", pos)] = ys
             live[("f", pos)] = fpool.tile([P, NM, P], F32, name="f", tag="f")
 
-        def apply_norm(pos, h):
+        def apply_norm(pos, hb):
             f = live[("f", pos)]
-            y = live[("y", pos)][h]
+            y = live[("y", pos)][hb]
             sc = live[("sc", pos // 2)]
             sh = live[("sh", pos // 2)]
-            x = 2 * h + pos % 2
+            e = pos % 2
             for i in range(4):
+                m = 4 * hb + i
                 for l in range(2):
-                    nc.scalar.activation(out=f[:, 4 * h + i, T * l:T * l + T], in_=y[:, i, T * l:T * l + T],
-                                         func=ACT.Relu, bias=sh[:, x, i, l:l + 1], scale=sc[:, x, i, l:l + 1])
+                    nc.scalar.activation(out=f[:, m, T * l:T * l + T], in_=y[:, i, T * l:T * l + T],
+                                         func=ACT.Relu, bias=sh[:, e, m, l:l + 1], scale=sc[:, e, m, l:l + 1])
 
-        def send(x, pos, tile_):
-            j = order[pos]
-            dst = (out_0, out_1)[x][2 * j:2 * j + 2].rearrange("l (h p i) t -> p (l h) (i t)", h=2, i=4)
-            src = tile_[:].rearrange("p l (h i) t -> p (l h) (i t)", h=2)
-            if j >= N_LATE or held[x] is None:
+        def send(x, dst, src):
+            if held[x] is None:
                 nc.sync.dma_start(out=dst, in_=src)
             else:
                 held[x].append((dst, src))
@@ -323,107 +303,117 @@ def tile_coarsepyramid_pa_kernel(tc, feature, segments, w_lr, b_lr, g_lr, be_lr,
                 nc.sync.dma_start(out=dst, in_=src)
             held[x] = None
 
-        def out_tile(pos, name):
-            if order[pos] < N_LATE:
-                return late.tile([P, 2, NM, T], F32, name=name + "_late", tag=name + "_late")
-            return opool.tile([P, 2, NM, T], F32, name=name, tag=name)
-
         def store_feat(pos):
-            f2 = out_tile(pos, "f2")
-            nc.scalar.copy(out=f2[:], in_=live[("f", pos)][:].rearrange("p m (l t) -> p l m t", l=2))
-            send(0, pos, f2)
-
-        def level(pos, k):
-            if k == 0:
-                return live[("f", pos)][:].rearrange("p m (l t) -> p m l t", l=2)
-            return tab[:, k - 1, :, 0:2 * L_STEP[k]].rearrange("p m (l t) -> p m l t", l=2)
+            j = order[pos]
+            is_late = j < SLOT_B // 2
+            f = live[("f", pos)]
+            if is_late:
+                f2 = late.tile([P, 2, NM, T], F32, name="f2_late", tag="f2_late")
+            else:
+                f2 = opool.tile([P, 2, NM, T], F32, name="f2", tag="f2")
+            nc.scalar.copy(out=f2[:], in_=f[:].rearrange("p m (l t) -> p l m t", l=2))
+            dst = out_0[2 * j:2 * j + 2].rearrange("l (p m) t -> p l (m t)", m=NM)
+            if is_late:
+                send(0, dst, f2[:].rearrange("p l m t -> p l (m t)"))
+            else:
+                nc.sync.dma_start(out=dst, in_=f2[:].rearrange("p l m t -> p l (m t)"))
 
         def level_up(pos, k):
             s = 2 ** k
             n_ok = T - 2 * s + 1
-            prev = level(pos, k)
-            nc.vector.tensor_tensor(out=level(pos, k + 1)[:, :, :, 0:n_ok], in0=prev[:, :, :, 0:n_ok],
-                                    in1=prev[:, :, :, s:s + n_ok], op=ALU.max)
+            if k == 0:
+                prev = live[("f", pos)][:].rearrange("p m (l t) -> p (m l) t", l=2)
+            else:
+                prev = tab[:, k - 1, :, :].rearrange("p m (l t) -> p (m l) t", l=2)
+            nxt = tab[:, k, :, :].rearrange("p m (l t) -> p (m l) t", l=2)
+            nc.vector.tensor_tensor(out=nxt[:, :, 0:n_ok], in0=prev[:, :, 0:n_ok], in1=prev[:, :, s:s + n_ok], op=ALU.max)
 
         def rows_out(pos, k):
+            f = live[("f", pos)]
             if k == 0:
-                live[("r", pos)] = rpool.tile([P, LEV, 2, C], F32, name="r", tag="r")
+                live[("r", pos)] = rpool.tile([P, LEV, 2, NM, 64], F32, name="r", tag="r")
             r = live[("r", pos)]
-            for h in range(2):
+            for hb in range(2):
                 tp = tpsum.tile([P, 4, P], F32, tag="tp")
                 for i in range(4):
-                    m = 4 * h + i
-                    src = live[("f", pos)][:, m, :] if k == 0 else tab[:, k - 1, m, :]
+                    m = 4 * hb + i
+                    src = f[:, m, :] if k == 0 else tab[:, k - 1, m, :]
                     nc.tensor.transpose(tp[:, i, :], src, ident[:])
+                dst = r[:, k, :, 4 * hb:4 * hb + 4, :]
+                view = tp[:].rearrange("p m (h q) -> p h m q", h=2)
                 if k >= 4:
-                    nc.vector.tensor_copy(out=r[:, k, h, :], in_=tp[:].rearrange("p i q -> p (i q)"))
+                    nc.vector.tensor_copy(out=dst, in_=view)
                 else:
-                    nc.scalar.copy(out=r[:, k, h, :], in_=tp[:].rearrange("p i q -> p (i q)"))
-            slot = slot_wide[pos % 2]
-            if k in (1, 3):
-                nc.sync.dma_start(out=slot[ROW0[k - 1]:ROW0[k - 1] + 2 * P, :].rearrange("(k r) w -> r k w", k=2),
-                                  in_=r[:, k - 1:k + 1, :, :].rearrange("p k h c -> p k (h c)"))
-            if k >= 4:
-                n_r = 2 * L_STEP[k]
-                nc.sync.dma_start(out=slot[ROW0[k]:ROW0[k] + n_r, :], in_=r[0:n_r, k, :, :].rearrange("p h c -> p (h c)"))
+                    nc.scalar.copy(out=dst, in_=view)
+            if k % 2 == 1:
+                nc.sync.dma_start(out=slot_store[pos % 2][:, k - 1:k + 1, :],
+                                  in_=r[:, k - 1:k + 1, :, :, :].rearrange("p k h m q -> p k (h m q)"))
 
         def gathers(pos):
             j = order[pos]
             got = []
             for h in range(2):
-                pair = []
-                for e in range(2):
-                    ga = gpool.tile([P, C], F32, name="g%d%d" % (h, e), tag="g%d%d" % (h, e))
-                    nc.gpsimd.indirect_dma_start(out=ga[:], out_offset=None, in_=slot_rows[pos % 2],
-                                                 in_offset=bass.IndirectOffsetOnAxis(ap=idx[:, j, h, e:e + 1], axis=0))
-                    pair.append(ga)
-                got.append(pair)
+                ga = gpool.tile([P, C], F32, name="ga%d" % h, tag="ga%d" % h, bufs=3)
+                gb = gpool.tile([P, C], F32, name="gb%d" % h, tag="gb%d" % h, bufs=3)
+                nc.gpsimd.indirect_dma_start(out=ga[:], out_offset=None, in_=slot_rows[pos % 2],
+                                             in_offset=bass.IndirectOffsetOnAxis(ap=idx[:, j, h, 0:1], axis=0))
+                nc.gpsimd.indirect_dma_start(out=gb[:], out_offset=None, in_=slot_rows[pos % 2],
+                                             in_offset=bass.IndirectOffsetOnAxis(ap=idx[:, j, h, 1:2], axis=0))
+                got.append((ga, gb))
             live[("g", pos)] = got
 
-        def pooled_turn(pos, h):
-            banks = []
-            for e in range(2):
-                bank = opsum.tile([P, 4, P], F32, name="bank", tag="op")
-                for i in range(4):
-                    nc.tensor.transpose(bank[:, i, :], live[("g", pos)][h][e][:, P * i:P * i + P], ident[:])
-                banks.append(bank)
-                if e == 0:
-                    one = opool.tile([P, 4, P], F32, name="one", tag="one")
-                    nc.scalar.copy(out=one[:], in_=bank[:])
-            live[("turn", pos, h)] = (one, banks[1])
+        def window_max(pos):
+            gc = gpool.tile([P, NM, 2, 64], F32)
+            for h in range(2):
+                ga, gb = live[("g", pos)][h]
+                nc.vector.tensor_tensor(out=gc[:, :, h, :], in0=ga[:].rearrange("p (m q) -> p m q", m=NM),
+                                        in1=gb[:].rearrange("p (m q) -> p m q", m=NM), op=ALU.max)
+            live[("gc", pos)] = gc
 
-        def pooled_max(pos, h):
-            if h == 0:
-                live[("o", pos)] = out_tile(pos, "o")
+        def pooled_out(pos, hb):
+            j = order[pos]
+            is_late = j < SLOT_B // 2
+            gc = live[("gc", pos)]
+            if hb == 0:
+                if is_late:
+                    live[("o", pos)] = late.tile([P, 2, NM, T], F32, name="o_late", tag="o_late")
+                else:
+                    live[("o", pos)] = opool.tile([P, 2, NM, T], F32, name="o", tag="o")
             o = live[("o", pos)]
-            one, bank = live[("turn", pos, h)]
-            nc.vector.tensor_tensor(out=o[:, :, 4 * h:4 * h + 4, :], in0=bank[:].rearrange("p i (l n) -> p l i n", l=2),
-                                    in1=one[:].rearrange("p i (l n) -> p l i n", l=2), op=ALU.max)
-            if h == 1:
-                send(1, pos, o)
+            op = opsum.tile([P, 4, P], F32, tag="op")
+            for i in range(4):
+                nc.tensor.transpose(op[:, i, :], gc[:, 4 * hb + i, :, :].rearrange("p h q -> p (h q)"), ident[:])
+            nc.scalar.copy(out=o[:, :, 4 * hb:4 * hb + 4, :], in_=op[:].rearrange("p m (l n) -> p l m n", l=2))
+            if hb == 1:
+                dst = out_1[2 * j:2 * j + 2].rearrange("l (p m) n -> p l (m n)", m=NM)
+                if is_late:
+                    send(1, dst, o[:].rearrange("p l m n -> p l (m n)"))
+                else:
+                    nc.sync.dma_start(out=dst, in_=o[:].rearrange("p l m n -> p l (m n)"))
 
         for pos in range(2):
-            for h in range(2):
-                sums_mx(pos, h)
-                sums(pos, h)
+            for hb in range(2):
+                sums_mx(pos, hb)
+                sums(pos, hb)
         chain_a(0)
         chain_b(0)
         chain_c(0)
-        for a in range(NCH + 3):
+        for a in range(NCH + 4):
             first = a < NCH
             second = 0 <= a - 1 < NCH
             third = 0 <= a - 3 < NCH
+            fourth = 0 <= a - 4 < NCH
             g_next = (a + 1) // 2 if a % 2 == 1 else NCH
             for q in range(2, len(pieces)):
                 if first_use(q) - 6 == a:
                     load_piece(q)
+            if fourth:
+                pooled_out(a - 4, 0)
             if second:
                 rows_out(a - 1, 0)
                 level_up(a - 1, 0)
             if first:
                 main_mx(a)
-            if third:
-                pooled_turn(a - 3, 0)
             if second:
                 level_up(a - 1, 1)
                 rows_out(a - 1, 1)
@@ -432,36 +422,34 @@ def tile_coarsepyramid_pa_kernel(tc, feature, segments, w_lr, b_lr, g_lr, be_lr,
                 apply_norm(a, 1)
                 store_feat(a)
                 quantise_piece(1)
-                for h in range(2):
-                    sums_mx(2, h)
-                    sums(2, h)
+                for hb in range(2):
+                    sums_mx(2, hb)
+                    sums(2, hb)
                 gather_indices()
+            sums_mx(a + 3, 0)
+            sums_mx(a + 3, 1)
             if second:
                 level_up(a - 1, 2)
                 rows_out(a - 1, 2)
                 level_up(a - 1, 3)
-            if third:
-                pooled_turn(a - 3, 1)
-            if second:
                 rows_out(a - 1, 3)
                 level_up(a - 1, 4)
                 rows_out(a - 1, 4)
                 rows_out(a - 1, 5)
                 gathers(a - 1)
-            if third:
-                pooled_max(a - 3, 0)
-                pooled_max(a - 3, 1)
-                if a - 3 >= NCH - 2:
-                    give_up_slot((a - 3) % 2)
             chain_a(g_next)
             if first and a > 0:
                 apply_norm(a, 0)
                 apply_norm(a, 1)
                 store_feat(a)
-            sums_mx(a + 3, 0)
-            sums_mx(a + 3, 1)
             sums(a + 3, 0)
             chain_b(g_next)
+            if third:
+                window_max(a - 3)
+                if a - 3 >= NCH - 2:
+                    give_up_slot((a - 3) % 2)
+            if fourth:
+                pooled_out(a - 4, 1)
             sums(a + 3, 1)
             chain_c(g_next)
             for q in range(2, len(pieces)):

@@ -68,59 +68,6 @@ def tile_coarsepyramid_pa_kernel(tc, feature, segments, w_lr, b_lr, g_lr, be_lr,
         ident = const.tile([P, P], F32)
         tab = const.tile([P, LEV - 1, NM, P], F32)
         pid_i = const.tile([P, 1], I32)
-        with tc.tile_pool(name="wstage", bufs=1) as wstage:
-            w_sb = wstage.tile([P, NM, C], BF16)
-            nc.sync.dma_start(out=w_sb[:], in_=w_lr.rearrange("(p m) k -> p m k", m=NM))
-            load_piece(0)
-            load_piece(1)
-            for i, v in enumerate((b_lr, g_lr, be_lr)):
-                nc.scalar.dma_start(out=vec_bf[i][:], in_=v.rearrange("(p m) -> p m", m=NM))
-            nc.scalar.dma_start(out=seg_bf[:], in_=segments.rearrange("(j l) n s -> (l n) j s", l=2))
-            make_identity(nc, ident[:])
-            nc.gpsimd.iota(pid_i[:], pattern=[[0, 1]], base=0, channel_multiplier=1)
-            nc.gpsimd.memset(tab[:], 0.0)
-
-            w_words = w_sb[:].bitcast(F32).rearrange("p m (q u) -> p m q u", u=2)
-            w_grp = wstage.tile([P, NM, P, 4], BF16, align_bytes=64)
-            w_grp32 = w_grp[:].bitcast(F32)
-            for mp in range(NM // 2):
-                wt = tpsum.tile([P, 4, P], F32, tag="tp")
-                for i in range(2):
-                    for u in range(2):
-                        nc.tensor.transpose(wt[:, 2 * i + u, :], w_words[:, 2 * mp + i, :, u], ident[:])
-                nc.vector.tensor_copy(out=w_grp32[:, 2 * mp, :, :], in_=wt[:, 0:2, :].rearrange("p u r -> p r u"))
-                nc.scalar.copy(out=w_grp32[:, 2 * mp + 1, :, :], in_=wt[:, 2:4, :].rearrange("p u r -> p r u"))
-            nc.vector.quantize_mx(out=w_codes[:].rearrange("p m c -> p (m c)").bitcast(FP8X4),
-                                  scales=w_scales[:].rearrange("p m c -> p (m c)"),
-                                  in_=w_grp[:].rearrange("p m c j -> p (m c j)"))
-        quantise_piece(0)
-
-        grp = const.tile([P, 32], F32)
-        nc.vector.tensor_reduce(out=grp[:], in_=ident[:].rearrange("p (q r) -> p q r", r=4), axis=AX.X, op=ALU.add)
-        bd = const.tile([P, 32, 4], F32)
-        nc.vector.tensor_scalar(out=bd[:], in0=grp[:].unsqueeze(2).to_broadcast([P, 32, 4]),
-                                scalar1=1.0 / 2048.0, scalar2=None, op0=ALU.mult)
-        bd2 = bd[:].rearrange("p q r -> p (q r)")
-        vec = const.tile([P, 3, NM], F32)
-        for i in range(3):
-            nc.vector.tensor_copy(out=vec[:, i, :], in_=vec_bf[i][:])
-        beta = vec[:, 0, :]
-        gamma = vec[:, 1, :]
-        shift0 = vec[:, 2, :]
-        beta2 = const.tile([P, NM], F32)
-        nc.vector.tensor_scalar(out=beta2[:], in0=beta, scalar1=2.0, scalar2=None, op0=ALU.mult)
-        bsq = const.tile([P, NM], F32)
-        nc.vector.tensor_tensor(out=bsq[:], in0=beta, in1=beta, op=ALU.mult)
-        cc = const.tile([P, 2], F32)
-        nc.vector.tensor_reduce(out=cc[:, 0:1], in_=beta, axis=AX.X, op=ALU.add)
-        nc.vector.tensor_reduce(out=cc[:, 1:2], in_=bsq[:], axis=AX.X, op=ALU.add)
-        cc64 = const.tile([P, 2], F32)
-        nc.vector.tensor_scalar(out=cc64[:], in0=cc[:], scalar1=64.0, scalar2=None, op0=ALU.mult)
-        cg_ps = opsum.tile([P, 2], F32, tag="op")
-        nc.tensor.matmul(out=cg_ps[:], lhsT=bd2, rhs=cc64[:], start=True, stop=True)
-        cg = const.tile([P, 2], F32)
-        nc.vector.tensor_copy(out=cg[:], in_=cg_ps[:])
-
         idx = const.tile([P, NCH, 2, 2], I32)
 
         def gather_indices():
@@ -175,6 +122,66 @@ def tile_coarsepyramid_pa_kernel(tc, feature, segments, w_lr, b_lr, g_lr, be_lr,
             nc.vector.tensor_scalar(out=rows4[:, :, 1, :], in0=rows4[:, :, 1, :], scalar1=1.0, scalar2=None, op0=ALU.add)
             nc.vector.tensor_copy(out=idx[:].rearrange("p j h e -> p (j h e)"), in_=rows[:].rearrange("p q e -> p (q e)"))
 
+
+        with tc.tile_pool(name="wstage", bufs=1) as wstage:
+            w_sb = wstage.tile([P, NM, C], BF16)
+            nc.scalar.dma_start(out=seg_bf[:], in_=segments.rearrange("(j l) n s -> (l n) j s", l=2))
+            for mp in range(NM // 2):
+                nc.sync.dma_start(out=w_sb[:, 2 * mp:2 * mp + 2, :],
+                                  in_=w_lr.rearrange("(p m) k -> p m k", m=NM)[:, 2 * mp:2 * mp + 2, :])
+                if mp == 0:
+                    load_piece(0)
+            load_piece(1)
+            for i, v in enumerate((b_lr, g_lr, be_lr)):
+                nc.scalar.dma_start(out=vec_bf[i][:], in_=v.rearrange("(p m) -> p m", m=NM))
+            make_identity(nc, ident[:])
+            nc.gpsimd.iota(pid_i[:], pattern=[[0, 1]], base=0, channel_multiplier=1)
+            nc.gpsimd.memset(tab[:], 0.0)
+            gather_indices()
+
+            w_words = w_sb[:].bitcast(F32).rearrange("p m (q u) -> p m q u", u=2)
+            w_grp = wstage.tile([P, NM, P, 4], BF16, align_bytes=64)
+            w_grp32 = w_grp[:].bitcast(F32)
+            for mp in range(NM // 2):
+                wt = tpsum.tile([P, 4, P], F32, tag="tp")
+                for i in range(2):
+                    for u in range(2):
+                        nc.tensor.transpose(wt[:, 2 * i + u, :], w_words[:, 2 * mp + i, :, u], ident[:])
+                nc.scalar.copy(out=w_grp32[:, 2 * mp, :, :], in_=wt[:, 0:2, :].rearrange("p u r -> p r u"))
+                nc.scalar.copy(out=w_grp32[:, 2 * mp + 1, :, :], in_=wt[:, 2:4, :].rearrange("p u r -> p r u"))
+                if mp == 0:
+                    quantise_piece(0)
+                if mp % 2 == 1:
+                    ms = slice(2 * mp - 2, 2 * mp + 2)
+                    nc.vector.quantize_mx(out=w_codes[:, ms, :].rearrange("p m c -> p (m c)").bitcast(FP8X4),
+                                          scales=w_scales[:, ms, :].rearrange("p m c -> p (m c)"),
+                                          in_=w_grp[:, ms, :, :].rearrange("p m c j -> p (m c j)"))
+
+        grp = const.tile([P, 32], F32)
+        nc.vector.tensor_reduce(out=grp[:], in_=ident[:].rearrange("p (q r) -> p q r", r=4), axis=AX.X, op=ALU.add)
+        bd = const.tile([P, 32, 4], F32)
+        nc.vector.tensor_scalar(out=bd[:], in0=grp[:].unsqueeze(2).to_broadcast([P, 32, 4]),
+                                scalar1=1.0 / 2048.0, scalar2=None, op0=ALU.mult)
+        bd2 = bd[:].rearrange("p q r -> p (q r)")
+        vec = const.tile([P, 3, NM], F32)
+        for i in range(3):
+            nc.vector.tensor_copy(out=vec[:, i, :], in_=vec_bf[i][:])
+        beta = vec[:, 0, :]
+        gamma = vec[:, 1, :]
+        shift0 = vec[:, 2, :]
+        beta2 = const.tile([P, NM], F32)
+        nc.vector.tensor_scalar(out=beta2[:], in0=beta, scalar1=2.0, scalar2=None, op0=ALU.mult)
+        bsq = const.tile([P, NM], F32)
+        nc.vector.tensor_tensor(out=bsq[:], in0=beta, in1=beta, op=ALU.mult)
+        cc = const.tile([P, 2], F32)
+        nc.vector.tensor_reduce(out=cc[:, 0:1], in_=beta, axis=AX.X, op=ALU.add)
+        nc.vector.tensor_reduce(out=cc[:, 1:2], in_=bsq[:], axis=AX.X, op=ALU.add)
+        cc64 = const.tile([P, 2], F32)
+        nc.vector.tensor_scalar(out=cc64[:], in0=cc[:], scalar1=64.0, scalar2=None, op0=ALU.mult)
+        cg_ps = opsum.tile([P, 2], F32, tag="op")
+        nc.tensor.matmul(out=cg_ps[:], lhsT=bd2, rhs=cc64[:], start=True, stop=True)
+        cg = const.tile([P, 2], F32)
+        nc.vector.tensor_copy(out=cg[:], in_=cg_ps[:])
 
         fpool = ctx.enter_context(tc.tile_pool(name="fpool", bufs=2))
         late = ctx.enter_context(tc.tile_pool(name="late", bufs=6))
@@ -414,6 +421,8 @@ def tile_coarsepyramid_pa_kernel(tc, feature, segments, w_lr, b_lr, g_lr, be_lr,
                 level_up(a - 1, 0)
             if first:
                 main_mx(a)
+            if a == 1:
+                quantise_piece(1)
             if second:
                 level_up(a - 1, 1)
                 rows_out(a - 1, 1)
@@ -421,13 +430,9 @@ def tile_coarsepyramid_pa_kernel(tc, feature, segments, w_lr, b_lr, g_lr, be_lr,
                 apply_norm(a, 0)
                 apply_norm(a, 1)
                 store_feat(a)
-                quantise_piece(1)
-                for hb in range(2):
-                    sums_mx(2, hb)
-                    sums(2, hb)
-                gather_indices()
-            sums_mx(a + 3, 0)
-            sums_mx(a + 3, 1)
+            if a > 0:
+                sums_mx(a + 3, 0)
+                sums_mx(a + 3, 1)
             if second:
                 level_up(a - 1, 2)
                 rows_out(a - 1, 2)
@@ -437,12 +442,20 @@ def tile_coarsepyramid_pa_kernel(tc, feature, segments, w_lr, b_lr, g_lr, be_lr,
                 rows_out(a - 1, 4)
                 rows_out(a - 1, 5)
                 gathers(a - 1)
+            if a == 1:
+                sums(a + 3, 0)
+                sums(a + 3, 1)
+                for pos in (2, 3):
+                    for hb in range(2):
+                        sums_mx(pos, hb)
+                        sums(pos, hb)
             chain_a(g_next)
             if first and a > 0:
                 apply_norm(a, 0)
                 apply_norm(a, 1)
                 store_feat(a)
-            sums(a + 3, 0)
+            if a > 1:
+                sums(a + 3, 0)
             chain_b(g_next)
             if third:
                 window_max(a - 3)
@@ -450,7 +463,8 @@ def tile_coarsepyramid_pa_kernel(tc, feature, segments, w_lr, b_lr, g_lr, be_lr,
                     give_up_slot((a - 3) % 2)
             if fourth:
                 pooled_out(a - 4, 1)
-            sums(a + 3, 1)
+            if a > 1:
+                sums(a + 3, 1)
             chain_c(g_next)
             for q in range(2, len(pieces)):
                 if first_use(q) - 4 == a:

@@ -26,6 +26,8 @@ FLOPS = 2 * B * C2 * C * T
 
 def tile_coarsepyramid_pa_kernel(tc, feature, segments, w_lr, b_lr, g_lr, be_lr, out_0, out_1):
     nc = tc.nc
+    N_OK = [T - 2 ** k + 1 for k in range(LEV)]
+    STORED = [P, P, P, P, 112, 80]
     with ExitStack() as ctx:
         const = ctx.enter_context(tc.tile_pool(name="const", bufs=1))
         small = ctx.enter_context(tc.tile_pool(name="small", bufs=3))
@@ -100,24 +102,30 @@ def tile_coarsepyramid_pa_kernel(tc, feature, segments, w_lr, b_lr, g_lr, be_lr,
                 nc.vector.scalar_tensor_tensor(out=lev256[:], in0=step[:], scalar=2.0, in1=lev256[:], op0=ALU.mult, op1=ALU.add)
                 nc.vector.scalar_tensor_tensor(out=wid[:], in0=step[:], scalar=float(2 ** (k - 1)), in1=wid[:], op0=ALU.mult, op1=ALU.add)
             low_i = const.tile([P, 1], I32)
-            nc.vector.tensor_single_scalar(out=low_i[:], in_=pid_i[:], scalar=15, op=ALU.bitwise_and)
+            nc.vector.tensor_single_scalar(out=low_i[:], in_=pid_i[:], scalar=31, op=ALU.bitwise_and)
             pid = const.tile([P, 1], F32)
             nc.vector.tensor_copy(out=pid[:], in_=pid_i[:])
             low = const.tile([P, 1], F32)
             nc.vector.tensor_copy(out=low[:], in_=low_i[:])
-            lbase = const.tile([P, 1], F32)
-            nc.vector.tensor_scalar(out=lbase[:], in0=pid[:], scalar1=64.0, scalar2=768.0, op0=ALU.is_ge, op1=ALU.mult)
+            second = const.tile([P, 1], F32)
+            nc.vector.tensor_scalar(out=second[:], in0=pid[:], scalar1=64.0, scalar2=None, op0=ALU.is_ge)
             zrow = const.tile([P, 1], F32)
-            nc.vector.tensor_scalar(out=zrow[:], in0=low[:], scalar1=12.0, scalar2=float(12 * 48 + 2 * 5), op0=ALU.mult, op1=ALU.add)
+            nc.vector.tensor_scalar(out=zrow[:], in0=low[:], scalar1=12.0, scalar2=float(12 * STORED[5] + 2 * 5), op0=ALU.mult, op1=ALU.add)
+            nl = const.tile([P, NQ], F32)
+            nc.vector.tensor_scalar(out=nl[:], in0=wid[:], scalar1=-1.0, scalar2=float(T), op0=ALU.mult, op1=ALU.add)
+            nc.vector.tensor_scalar(out=nl[:], in0=nl[:], scalar1=second[:, 0:1], scalar2=None, op0=ALU.mult)
             rows = const.tile([P, NQ, 2], F32)
-            nc.vector.scalar_tensor_tensor(out=rows[:, :, 0], in0=lo, scalar=12.0, in1=lev256[:], op0=ALU.mult, op1=ALU.add)
+            t1 = const.tile([P, NQ], F32)
+            nc.vector.tensor_tensor(out=t1[:], in0=lo, in1=nl[:], op=ALU.add)
+            nc.vector.scalar_tensor_tensor(out=rows[:, :, 0], in0=t1[:], scalar=12.0, in1=lev256[:], op0=ALU.mult, op1=ALU.add)
             t2 = const.tile([P, NQ], F32)
             nc.vector.tensor_tensor(out=t2[:], in0=hi, in1=wid[:], op=ALU.subtract)
+            nc.vector.tensor_tensor(out=t2[:], in0=t2[:], in1=nl[:], op=ALU.add)
             nc.vector.scalar_tensor_tensor(out=rows[:, :, 1], in0=t2[:], scalar=12.0, in1=lev256[:], op0=ALU.mult, op1=ALU.add)
             for e in range(2):
                 nc.vector.tensor_scalar(out=rows[:, :, e], in0=rows[:, :, e], scalar1=zrow[:, 0:1], scalar2=None, op0=ALU.subtract)
                 nc.vector.tensor_tensor(out=rows[:, :, e], in0=rows[:, :, e], in1=valid[:], op=ALU.mult)
-                nc.vector.tensor_scalar(out=rows[:, :, e], in0=rows[:, :, e], scalar1=zrow[:, 0:1], scalar2=lbase[:, 0:1], op0=ALU.add, op1=ALU.add)
+                nc.vector.tensor_scalar(out=rows[:, :, e], in0=rows[:, :, e], scalar1=zrow[:, 0:1], scalar2=None, op0=ALU.add)
             rows4 = rows[:].rearrange("p (j h) e -> p j h e", h=2)
             nc.vector.tensor_scalar(out=rows4[:, :, 1, :], in0=rows4[:, :, 1, :], scalar1=1.0, scalar2=None, op0=ALU.add)
             nc.vector.tensor_copy(out=idx[:].rearrange("p j h e -> p (j h e)"), in_=rows[:].rearrange("p q e -> p (q e)"))
@@ -193,6 +201,9 @@ def tile_coarsepyramid_pa_kernel(tc, feature, segments, w_lr, b_lr, g_lr, be_lr,
         slot_store = [o[0:SLOT_B].rearrange("b (x c) t -> (b x) (c t)", c=16).rearrange("(r k) w -> r k w", k=LEV)
                       for o in slots]
         slot_rows = [o[0:SLOT_B].rearrange("b (x c) t -> (b x) (c t)", c=8) for o in slots]
+        for x in range(2):
+            for k in (4, 5):
+                nc.scalar.dma_start(out=slot_store[x][STORED[k]:P, k, :], in_=tab[STORED[k]:P, 0, :, :].rearrange("p m c -> p (m c)"))
 
         def mx_passes(y, pos, hb):
             cols = slice(P * order[pos], P * order[pos] + P)
@@ -327,13 +338,13 @@ def tile_coarsepyramid_pa_kernel(tc, feature, segments, w_lr, b_lr, g_lr, be_lr,
 
         def level_up(pos, k):
             s = 2 ** k
-            n_ok = T - 2 * s + 1
+            n_ok = N_OK[k + 1]
             if k == 0:
-                prev = live[("f", pos)][:].rearrange("p m (l t) -> p (m l) t", l=2)
+                prev = live[("f", pos)][:].rearrange("p m (l t) -> p m l t", l=2)
             else:
-                prev = tab[:, k - 1, :, :].rearrange("p m (l t) -> p (m l) t", l=2)
-            nxt = tab[:, k, :, :].rearrange("p m (l t) -> p (m l) t", l=2)
-            nc.vector.tensor_tensor(out=nxt[:, :, 0:n_ok], in0=prev[:, :, 0:n_ok], in1=prev[:, :, s:s + n_ok], op=ALU.max)
+                prev = tab[:, k - 1, :, 0:2 * N_OK[k]].rearrange("p m (l t) -> p m l t", l=2)
+            nxt = tab[:, k, :, 0:2 * n_ok].rearrange("p m (l t) -> p m l t", l=2)
+            nc.vector.tensor_tensor(out=nxt, in0=prev[:, :, :, 0:n_ok], in1=prev[:, :, :, s:s + n_ok], op=ALU.max)
 
         def rows_out(pos, k):
             f = live[("f", pos)]
@@ -352,9 +363,12 @@ def tile_coarsepyramid_pa_kernel(tc, feature, segments, w_lr, b_lr, g_lr, be_lr,
                     nc.vector.tensor_copy(out=dst, in_=view)
                 else:
                     nc.scalar.copy(out=dst, in_=view)
-            if k % 2 == 1:
+            if k in (1, 3):
                 nc.sync.dma_start(out=slot_store[pos % 2][:, k - 1:k + 1, :],
                                   in_=r[:, k - 1:k + 1, :, :, :].rearrange("p k h m q -> p k (h m q)"))
+            if k >= 4:
+                nc.sync.dma_start(out=slot_store[pos % 2][0:STORED[k], k:k + 1, :],
+                                  in_=r[0:STORED[k], k:k + 1, :, :, :].rearrange("p k h m q -> p k (h m q)"))
 
         def gathers(pos):
             j = order[pos]

@@ -58,7 +58,7 @@ def tile_coarsepyramid_pa_kernel(tc, feature, segments, w_lr, b_lr, g_lr, be_lr,
             b0, nb = pieces[q]
             raw = live[("raw", q)]
             x_grp = stage.tile([P, 8, T, 4], BF16, align_bytes=64, name="x_grp", tag="x_grp")
-            nc.vector.tensor_copy(out=x_grp[:, 0:nb, :, :], in_=raw[:, 0:nb, :, :].rearrange("p b j t -> p b t j"))
+            nc.scalar.copy(out=x_grp[:, 0:nb, :, :], in_=raw[:, 0:nb, :, :].rearrange("p b j t -> p b t j"))
             nc.vector.quantize_mx(out=x_codes[:, T * b0:T * (b0 + nb)].bitcast(FP8X4),
                                   scales=x_scales[:, T * b0:T * (b0 + nb)],
                                   in_=x_grp[:, 0:nb, :, :].rearrange("p b t j -> p (b t j)"))

@@ -18,16 +18,19 @@ P = 128
 B, C, T, C2 = 48, 512, 64, 1024
 NM = 8
 NCH = B // 2
-LEV = 6
+SIZES = [1, 3, 6, 12, 24, 48]
+LEV = len(SIZES)
+TAB = 5
 EPS = 1e-5
-SLOT_B = 12
+SLOT_B = 10
 FLOPS = 2 * B * C2 * C * T
 
 
 def tile_coarsepyramid_pa_kernel(tc, feature, segments, w_lr, b_lr, g_lr, be_lr, out_0, out_1):
     nc = tc.nc
-    N_OK = [T - 2 ** k + 1 for k in range(LEV)]
-    STORED = [P, P, P, P, 112, 80]
+    N_OK = [T - w + 1 for w in SIZES]
+    TOP = 2 * N_OK[4]
+    ZERO = TOP + 2 * N_OK[5]
     with ExitStack() as ctx:
         const = ctx.enter_context(tc.tile_pool(name="const", bufs=1))
         small = ctx.enter_context(tc.tile_pool(name="small", bufs=3))
@@ -40,7 +43,7 @@ def tile_coarsepyramid_pa_kernel(tc, feature, segments, w_lr, b_lr, g_lr, be_lr,
         live = {}
         held = {0: [], 1: []}
 
-        pieces = [(12, 4), (16, 8), (24, 8), (32, 8), (40, 8), (0, 8), (8, 4)]
+        pieces = [(10, 4), (14, 8), (22, 8), (30, 8), (38, 8), (46, 2), (0, 8), (8, 2)]
         x_codes = const.tile([P, B * T], U32, align_bytes=64)
         x_scales = const.tile([P, B * T], U8, align_bytes=64)
 
@@ -68,7 +71,8 @@ def tile_coarsepyramid_pa_kernel(tc, feature, segments, w_lr, b_lr, g_lr, be_lr,
         vec_bf = [const.tile([P, NM], BF16, name="vec_bf%d" % i) for i in range(3)]
         seg_bf = const.tile([P, NCH, 4], BF16)
         ident = const.tile([P, P], F32)
-        tab = const.tile([P, LEV - 1, NM, P], F32)
+        tab = const.tile([P, TAB - 1, NM, P], F32)
+        pairs = const.tile([P, NM, 2 * (T - 1)], F32)
         pid_i = const.tile([P, 1], I32)
         idx = const.tile([P, NCH, 2, 2], I32)
 
@@ -98,11 +102,12 @@ def tile_coarsepyramid_pa_kernel(tc, feature, segments, w_lr, b_lr, g_lr, be_lr,
             nc.vector.memset(wid[:], 0.0)
             step = const.tile([P, NQ], F32)
             for k in range(1, LEV):
-                nc.vector.tensor_scalar(out=step[:], in0=ln[:], scalar1=float(2 ** k), scalar2=None, op0=ALU.is_ge)
-                nc.vector.scalar_tensor_tensor(out=lev256[:], in0=step[:], scalar=2.0, in1=lev256[:], op0=ALU.mult, op1=ALU.add)
-                nc.vector.scalar_tensor_tensor(out=wid[:], in0=step[:], scalar=float(2 ** (k - 1)), in1=wid[:], op0=ALU.mult, op1=ALU.add)
+                off = 2.0 if k < TAB else float(2 * TAB * TOP)
+                nc.vector.tensor_scalar(out=step[:], in0=ln[:], scalar1=float(SIZES[k]), scalar2=None, op0=ALU.is_ge)
+                nc.vector.scalar_tensor_tensor(out=lev256[:], in0=step[:], scalar=off, in1=lev256[:], op0=ALU.mult, op1=ALU.add)
+                nc.vector.scalar_tensor_tensor(out=wid[:], in0=step[:], scalar=float(SIZES[k] - SIZES[k - 1]), in1=wid[:], op0=ALU.mult, op1=ALU.add)
             low_i = const.tile([P, 1], I32)
-            nc.vector.tensor_single_scalar(out=low_i[:], in_=pid_i[:], scalar=31, op=ALU.bitwise_and)
+            nc.vector.tensor_single_scalar(out=low_i[:], in_=pid_i[:], scalar=7, op=ALU.bitwise_and)
             pid = const.tile([P, 1], F32)
             nc.vector.tensor_copy(out=pid[:], in_=pid_i[:])
             low = const.tile([P, 1], F32)
@@ -110,18 +115,18 @@ def tile_coarsepyramid_pa_kernel(tc, feature, segments, w_lr, b_lr, g_lr, be_lr,
             second = const.tile([P, 1], F32)
             nc.vector.tensor_scalar(out=second[:], in0=pid[:], scalar1=64.0, scalar2=None, op0=ALU.is_ge)
             zrow = const.tile([P, 1], F32)
-            nc.vector.tensor_scalar(out=zrow[:], in0=low[:], scalar1=12.0, scalar2=float(12 * STORED[5] + 2 * 5), op0=ALU.mult, op1=ALU.add)
+            nc.vector.tensor_scalar(out=zrow[:], in0=low[:], scalar1=2.0 * TAB, scalar2=float(2 * TAB * ZERO + 2 * (TAB - 1)), op0=ALU.mult, op1=ALU.add)
             nl = const.tile([P, NQ], F32)
             nc.vector.tensor_scalar(out=nl[:], in0=wid[:], scalar1=-1.0, scalar2=float(T), op0=ALU.mult, op1=ALU.add)
             nc.vector.tensor_scalar(out=nl[:], in0=nl[:], scalar1=second[:, 0:1], scalar2=None, op0=ALU.mult)
             rows = const.tile([P, NQ, 2], F32)
             t1 = const.tile([P, NQ], F32)
             nc.vector.tensor_tensor(out=t1[:], in0=lo, in1=nl[:], op=ALU.add)
-            nc.vector.scalar_tensor_tensor(out=rows[:, :, 0], in0=t1[:], scalar=12.0, in1=lev256[:], op0=ALU.mult, op1=ALU.add)
+            nc.vector.scalar_tensor_tensor(out=rows[:, :, 0], in0=t1[:], scalar=2.0 * TAB, in1=lev256[:], op0=ALU.mult, op1=ALU.add)
             t2 = const.tile([P, NQ], F32)
             nc.vector.tensor_tensor(out=t2[:], in0=hi, in1=wid[:], op=ALU.subtract)
             nc.vector.tensor_tensor(out=t2[:], in0=t2[:], in1=nl[:], op=ALU.add)
-            nc.vector.scalar_tensor_tensor(out=rows[:, :, 1], in0=t2[:], scalar=12.0, in1=lev256[:], op0=ALU.mult, op1=ALU.add)
+            nc.vector.scalar_tensor_tensor(out=rows[:, :, 1], in0=t2[:], scalar=2.0 * TAB, in1=lev256[:], op0=ALU.mult, op1=ALU.add)
             for e in range(2):
                 nc.vector.tensor_scalar(out=rows[:, :, e], in0=rows[:, :, e], scalar1=zrow[:, 0:1], scalar2=None, op0=ALU.subtract)
                 nc.vector.tensor_tensor(out=rows[:, :, e], in0=rows[:, :, e], in1=valid[:], op=ALU.mult)
@@ -192,18 +197,15 @@ def tile_coarsepyramid_pa_kernel(tc, feature, segments, w_lr, b_lr, g_lr, be_lr,
         nc.vector.tensor_copy(out=cg[:], in_=cg_ps[:])
 
         fpool = ctx.enter_context(tc.tile_pool(name="fpool", bufs=2))
-        late = ctx.enter_context(tc.tile_pool(name="late", bufs=6))
+        late = ctx.enter_context(tc.tile_pool(name="late", bufs=5))
         rpool = ctx.enter_context(tc.tile_pool(name="rpool", bufs=2))
         gpool = ctx.enter_context(tc.tile_pool(name="gpool", bufs=2))
         opool = ctx.enter_context(tc.tile_pool(name="opool", bufs=2))
 
         slots = [out_0, out_1]
-        slot_store = [o[0:SLOT_B].rearrange("b (x c) t -> (b x) (c t)", c=16).rearrange("(r k) w -> r k w", k=LEV)
+        slot_store = [o[0:SLOT_B].rearrange("b (x c) t -> (b x) (c t)", c=16).rearrange("(r k) w -> r k w", k=TAB)
                       for o in slots]
         slot_rows = [o[0:SLOT_B].rearrange("b (x c) t -> (b x) (c t)", c=8) for o in slots]
-        for x in range(2):
-            for k in (4, 5):
-                nc.scalar.dma_start(out=slot_store[x][STORED[k]:P, k, :], in_=tab[STORED[k]:P, 0, :, :].rearrange("p m c -> p (m c)"))
 
         def mx_passes(y, pos, hb):
             cols = slice(P * order[pos], P * order[pos] + P)
@@ -336,20 +338,28 @@ def tile_coarsepyramid_pa_kernel(tc, feature, segments, w_lr, b_lr, g_lr, be_lr,
             else:
                 nc.sync.dma_start(out=dst, in_=f2[:].rearrange("p l m t -> p l (m t)"))
 
+        def view(k):
+            if k == 5:
+                cols = tab[:, 3, :, TOP:TOP + 2 * N_OK[5]]
+            else:
+                cols = tab[:, k - 1, :, 0:2 * N_OK[k]]
+            return cols.rearrange("p m (l t) -> p m l t", l=2)
+
         def level_up(pos, k):
-            s = 2 ** k
             n_ok = N_OK[k + 1]
             if k == 0:
-                prev = live[("f", pos)][:].rearrange("p m (l t) -> p m l t", l=2)
+                f = live[("f", pos)][:].rearrange("p m (l t) -> p m l t", l=2)
+                two = pairs[:].rearrange("p m (l t) -> p m l t", l=2)
+                nc.vector.tensor_tensor(out=two, in0=f[:, :, :, 0:T - 1], in1=f[:, :, :, 1:T], op=ALU.max)
+                prev, s = two, 1
             else:
-                prev = tab[:, k - 1, :, 0:2 * N_OK[k]].rearrange("p m (l t) -> p m l t", l=2)
-            nxt = tab[:, k, :, 0:2 * n_ok].rearrange("p m (l t) -> p m l t", l=2)
-            nc.vector.tensor_tensor(out=nxt, in0=prev[:, :, :, 0:n_ok], in1=prev[:, :, :, s:s + n_ok], op=ALU.max)
+                prev, s = view(k), SIZES[k]
+            nc.vector.tensor_tensor(out=view(k + 1), in0=prev[:, :, :, 0:n_ok], in1=prev[:, :, :, s:s + n_ok], op=ALU.max)
 
         def rows_out(pos, k):
             f = live[("f", pos)]
             if k == 0:
-                live[("r", pos)] = rpool.tile([P, LEV, 2, NM, 64], F32, name="r", tag="r")
+                live[("r", pos)] = rpool.tile([P, TAB, 2, NM, 64], F32, name="r", tag="r")
             r = live[("r", pos)]
             for hb in range(2):
                 tp = tpsum.tile([P, 4, P], F32, tag="tp")
@@ -358,17 +368,15 @@ def tile_coarsepyramid_pa_kernel(tc, feature, segments, w_lr, b_lr, g_lr, be_lr,
                     src = f[:, m, :] if k == 0 else tab[:, k - 1, m, :]
                     nc.tensor.transpose(tp[:, i, :], src, ident[:])
                 dst = r[:, k, :, 4 * hb:4 * hb + 4, :]
-                view = tp[:].rearrange("p m (h q) -> p h m q", h=2)
-                if k >= 4:
-                    nc.vector.tensor_copy(out=dst, in_=view)
+                rows = tp[:].rearrange("p m (h q) -> p h m q", h=2)
+                if k == TAB - 1:
+                    nc.vector.tensor_copy(out=dst, in_=rows)
                 else:
-                    nc.scalar.copy(out=dst, in_=view)
-            if k in (1, 3):
-                nc.sync.dma_start(out=slot_store[pos % 2][:, k - 1:k + 1, :],
-                                  in_=r[:, k - 1:k + 1, :, :, :].rearrange("p k h m q -> p k (h m q)"))
-            if k >= 4:
-                nc.sync.dma_start(out=slot_store[pos % 2][0:STORED[k], k:k + 1, :],
-                                  in_=r[0:STORED[k], k:k + 1, :, :, :].rearrange("p k h m q -> p k (h m q)"))
+                    nc.scalar.copy(out=dst, in_=rows)
+            if k != 0 and k != 2:
+                first = k - 1 if k < TAB - 1 else k
+                nc.sync.dma_start(out=slot_store[pos % 2][:, first:k + 1, :],
+                                  in_=r[:, first:k + 1, :, :, :].rearrange("p k h m q -> p k (h m q)"))
 
         def gathers(pos):
             j = order[pos]
@@ -454,7 +462,6 @@ def tile_coarsepyramid_pa_kernel(tc, feature, segments, w_lr, b_lr, g_lr, be_lr,
                 rows_out(a - 1, 3)
                 level_up(a - 1, 4)
                 rows_out(a - 1, 4)
-                rows_out(a - 1, 5)
                 gathers(a - 1)
             if a == 1:
                 sums(a + 3, 0)

@@ -2,7 +2,7 @@ from contextlib import ExitStack
 
 import concourse.bass as bass
 import concourse.mybir as mybir
-from concourse.masks import make_identity
+from concourse.masks import make_block_diagonal, make_identity
 
 F32 = mybir.dt.float32
 BF16 = mybir.dt.bfloat16
@@ -20,30 +20,31 @@ NM = 8
 NCH = B // 2
 SIZES = [1, 3, 6, 12, 24, 48]
 LEV = len(SIZES)
+N_OK = [T - w + 1 for w in SIZES]
 TAB = 5
+TOP = 2 * N_OK[4]
+ZERO = TOP + 2 * N_OK[5]
 EPS = 1e-5
 SLOT_B = 10
+LATE = SLOT_B // 2
 FLOPS = 2 * B * C2 * C * T
 
 
 def tile_coarsepyramid_pa_kernel(tc, feature, segments, w_lr, b_lr, g_lr, be_lr, out_0, out_1):
     nc = tc.nc
-    N_OK = [T - w + 1 for w in SIZES]
-    TOP = 2 * N_OK[4]
-    ZERO = TOP + 2 * N_OK[5]
     with ExitStack() as ctx:
         const = ctx.enter_context(tc.tile_pool(name="const", bufs=1))
         small = ctx.enter_context(tc.tile_pool(name="small", bufs=3))
         stage = ctx.enter_context(tc.tile_pool(name="stage", bufs=2))
         ypsum = ctx.enter_context(tc.psum_pool(name="ypsum", bufs=1))
-        tpsum = ctx.enter_context(tc.psum_pool(name="tpsum", bufs=3))
-        opsum = ctx.enter_context(tc.psum_pool(name="opsum", bufs=1))
+        tpsum = ctx.enter_context(tc.psum_pool(name="tpsum", bufs=4))
+        opsum = ctx.enter_context(tc.psum_pool(name="opsum", bufs=2))
 
-        order = list(range(SLOT_B // 2, NCH)) + list(range(SLOT_B // 2))
+        order = list(range(LATE, NCH)) + list(range(LATE))
         live = {}
         held = {0: [], 1: []}
 
-        pieces = [(10, 4), (14, 8), (22, 8), (30, 8), (38, 8), (46, 2), (0, 8), (8, 2)]
+        pieces = [(10, 4), (14, 4), (18, 4), (22, 8), (30, 8), (38, 8), (46, 2), (0, 8), (8, 2)]
         x_codes = const.tile([P, B * T], U32, align_bytes=64)
         x_scales = const.tile([P, B * T], U8, align_bytes=64)
 
@@ -52,16 +53,24 @@ def tile_coarsepyramid_pa_kernel(tc, feature, segments, w_lr, b_lr, g_lr, be_lr,
 
         def load_piece(q):
             b0, nb = pieces[q]
-            raw = stage.tile([P, 8, 4, T], BF16, name="raw", tag="raw", bufs=3)
+            raw = stage.tile([P, 8, 4, T], BF16, name="raw", tag="raw")
             nc.sync.dma_start(out=raw[:, 0:nb, :, :].rearrange("p b j t -> p b (j t)"),
                               in_=feature[b0:b0 + nb].rearrange("b (p j) t -> p b (j t)", j=4))
             live[("raw", q)] = raw
 
+        def group_piece(q, b):
+            raw = live[("raw", q)]
+            if b == 0:
+                live[("x_grp", q)] = stage.tile([P, 8, T, 4], BF16, align_bytes=64, name="x_grp", tag="x_grp")
+            x_grp = live[("x_grp", q)]
+            if q == 0:
+                nc.vector.tensor_copy(out=x_grp[:, b:b + 2, :, :], in_=raw[:, b:b + 2, :, :].rearrange("p b j t -> p b t j"))
+            else:
+                nc.scalar.copy(out=x_grp[:, b:b + 2, :, :], in_=raw[:, b:b + 2, :, :].rearrange("p b j t -> p b t j"))
+
         def quantise_piece(q):
             b0, nb = pieces[q]
-            raw = live[("raw", q)]
-            x_grp = stage.tile([P, 8, T, 4], BF16, align_bytes=64, name="x_grp", tag="x_grp")
-            nc.scalar.copy(out=x_grp[:, 0:nb, :, :], in_=raw[:, 0:nb, :, :].rearrange("p b j t -> p b t j"))
+            x_grp = live[("x_grp", q)]
             nc.vector.quantize_mx(out=x_codes[:, T * b0:T * (b0 + nb)].bitcast(FP8X4),
                                   scales=x_scales[:, T * b0:T * (b0 + nb)],
                                   in_=x_grp[:, 0:nb, :, :].rearrange("p b t j -> p (b t j)"))
@@ -69,141 +78,116 @@ def tile_coarsepyramid_pa_kernel(tc, feature, segments, w_lr, b_lr, g_lr, be_lr,
         w_codes = const.tile([P, NM, P], U32, align_bytes=64)
         w_scales = const.tile([P, NM, P], U8, align_bytes=64)
         vec_bf = [const.tile([P, NM], BF16, name="vec_bf%d" % i) for i in range(3)]
-        seg_bf = const.tile([P, NCH, 4], BF16)
+        beta, gamma, shift0 = [v[:] for v in vec_bf]
+        seg_bf = const.tile([P, NCH, 2, 2], BF16)
         ident = const.tile([P, P], F32)
-        tab = const.tile([P, TAB - 1, NM, P], F32)
-        pairs = const.tile([P, NM, 2 * (T - 1)], F32)
-        pid_i = const.tile([P, 1], I32)
+        ones4 = const.tile([P, P], F32)
+        tab = const.tile([P, TAB - 1, 2, 4, P], F32)
+        pairs = const.tile([P, 2, 4, 2 * (T - 1)], F32)
+        STEPS = [-1000.0, 0.0] + [float(w - 1) for w in SIZES[1:]]
+        NS = len(STEPS)
+        thr = const.tile([P, NS], F32)
+        gain = const.tile([P, 2, NS], F32)
         idx = const.tile([P, NCH, 2, 2], I32)
 
-        def gather_indices():
-            NQ = NCH * 2
-            sf = const.tile([P, NCH * 4], F32)
-            nc.vector.tensor_copy(out=sf[:], in_=seg_bf[:].rearrange("p j s -> p (j s)"))
-            nc.vector.tensor_scalar(out=sf[:], in0=sf[:], scalar1=0.0, scalar2=float(T - 1), op0=ALU.max, op1=ALU.min)
-            si = const.tile([P, NCH * 4], I32)
-            nc.vector.tensor_copy(out=si[:], in_=sf[:])
-            sr = const.tile([P, NCH * 4], F32)
-            nc.vector.tensor_copy(out=sr[:], in_=si[:])
-            over = const.tile([P, NCH * 4], F32)
-            nc.vector.tensor_tensor(out=over[:], in0=sr[:], in1=sf[:], op=ALU.is_gt)
-            fl = const.tile([P, NQ, 2], F32)
-            nc.vector.tensor_tensor(out=fl[:].rearrange("p q e -> p (q e)"), in0=sr[:], in1=over[:], op=ALU.subtract)
-            lo = fl[:, :, 0]
-            hi = fl[:, :, 1]
-            ln = const.tile([P, NQ], F32)
-            nc.vector.tensor_tensor(out=ln[:], in0=hi, in1=lo, op=ALU.subtract)
-            nc.vector.tensor_scalar(out=ln[:], in0=ln[:], scalar1=1.0, scalar2=None, op0=ALU.add)
-            valid = const.tile([P, NQ], F32)
-            nc.vector.tensor_scalar(out=valid[:], in0=ln[:], scalar1=1.0, scalar2=None, op0=ALU.is_ge)
-            lev256 = const.tile([P, NQ], F32)
-            wid = const.tile([P, NQ], F32)
-            nc.vector.memset(lev256[:], 0.0)
-            nc.vector.memset(wid[:], 0.0)
-            step = const.tile([P, NQ], F32)
-            for k in range(1, LEV):
-                off = 2.0 if k < TAB else float(2 * TAB * TOP)
-                nc.vector.tensor_scalar(out=step[:], in0=ln[:], scalar1=float(SIZES[k]), scalar2=None, op0=ALU.is_ge)
-                nc.vector.scalar_tensor_tensor(out=lev256[:], in0=step[:], scalar=off, in1=lev256[:], op0=ALU.mult, op1=ALU.add)
-                nc.vector.scalar_tensor_tensor(out=wid[:], in0=step[:], scalar=float(SIZES[k] - SIZES[k - 1]), in1=wid[:], op0=ALU.mult, op1=ALU.add)
-            low_i = const.tile([P, 1], I32)
-            nc.vector.tensor_single_scalar(out=low_i[:], in_=pid_i[:], scalar=7, op=ALU.bitwise_and)
-            pid = const.tile([P, 1], F32)
-            nc.vector.tensor_copy(out=pid[:], in_=pid_i[:])
-            low = const.tile([P, 1], F32)
-            nc.vector.tensor_copy(out=low[:], in_=low_i[:])
-            second = const.tile([P, 1], F32)
-            nc.vector.tensor_scalar(out=second[:], in0=pid[:], scalar1=64.0, scalar2=None, op0=ALU.is_ge)
-            zrow = const.tile([P, 1], F32)
-            nc.vector.tensor_scalar(out=zrow[:], in0=low[:], scalar1=2.0 * TAB, scalar2=float(2 * TAB * ZERO + 2 * (TAB - 1)), op0=ALU.mult, op1=ALU.add)
-            nl = const.tile([P, NQ], F32)
-            nc.vector.tensor_scalar(out=nl[:], in0=wid[:], scalar1=-1.0, scalar2=float(T), op0=ALU.mult, op1=ALU.add)
-            nc.vector.tensor_scalar(out=nl[:], in0=nl[:], scalar1=second[:, 0:1], scalar2=None, op0=ALU.mult)
-            rows = const.tile([P, NQ, 2], F32)
-            t1 = const.tile([P, NQ], F32)
-            nc.vector.tensor_tensor(out=t1[:], in0=lo, in1=nl[:], op=ALU.add)
-            nc.vector.scalar_tensor_tensor(out=rows[:, :, 0], in0=t1[:], scalar=2.0 * TAB, in1=lev256[:], op0=ALU.mult, op1=ALU.add)
-            t2 = const.tile([P, NQ], F32)
-            nc.vector.tensor_tensor(out=t2[:], in0=hi, in1=wid[:], op=ALU.subtract)
-            nc.vector.tensor_tensor(out=t2[:], in0=t2[:], in1=nl[:], op=ALU.add)
-            nc.vector.scalar_tensor_tensor(out=rows[:, :, 1], in0=t2[:], scalar=2.0 * TAB, in1=lev256[:], op0=ALU.mult, op1=ALU.add)
+        make_identity(nc, ident[:])
+        make_block_diagonal(nc, ones4[:], 4)
+        ctx.enter_context(tc.manual_schedule())
+
+        def step_constants():
+            for k in range(NS):
+                nc.vector.memset(thr[:, k:k + 1], STEPS[k])
+            for l in range(2):
+                for e in range(2):
+                    at = [5.0 * (ZERO + 4 * l + e) + TAB - 1]
+                    for k in range(LEV):
+                        row = l * N_OK[k] + (TOP if k == 5 else 0) - e * (SIZES[k] - 1)
+                        at.append(5.0 * row + min(k, TAB - 1))
+                    for k in range(NS):
+                        nc.vector.memset(gain[T * l:P, e, k:k + 1], at[k] - (at[k - 1] if k > 0 else 0.0))
+
+        NQ = NCH * 2
+        fl = const.tile([P, NCH, 2, 2], F32)
+        fl3 = fl[:].rearrange("p j h e -> p (j h) e")
+        ln = const.tile([P, NQ], F32)
+        step = const.tile([P, NS, NQ], F32)
+        part = const.tile([P, 2, NS, NQ], F32)
+
+        def window_ends():
+            whole = const.tile([P, NQ, 2], I32)
+            nc.vector.tensor_scalar(out=whole[:].rearrange("p q e -> p (q e)"), in0=seg_bf[:].rearrange("p j h e -> p (j h e)"),
+                                    scalar1=0.0, scalar2=-0.498, op0=ALU.max, op1=ALU.add)
+            for h in range(2):
+                nc.vector.tensor_scalar(out=fl[:, :, h, :], in0=whole[:].rearrange("p (j h) e -> p j h e", h=2)[:, :, h, :],
+                                        scalar1=float(T - 1), scalar2=128.0 * h, op0=ALU.min, op1=ALU.add)
+            nc.vector.tensor_tensor(out=ln[:], in0=fl3[:, :, 1], in1=fl3[:, :, 0], op=ALU.subtract)
+
+        def window_steps():
+            nc.vector.tensor_tensor(out=step[:], in0=ln[:].unsqueeze(1).to_broadcast([P, NS, NQ]),
+                                    in1=thr[:].unsqueeze(2).to_broadcast([P, NS, NQ]), op=ALU.is_ge)
             for e in range(2):
-                nc.vector.tensor_scalar(out=rows[:, :, e], in0=rows[:, :, e], scalar1=zrow[:, 0:1], scalar2=None, op0=ALU.subtract)
-                nc.vector.tensor_tensor(out=rows[:, :, e], in0=rows[:, :, e], in1=valid[:], op=ALU.mult)
-                nc.vector.tensor_scalar(out=rows[:, :, e], in0=rows[:, :, e], scalar1=zrow[:, 0:1], scalar2=None, op0=ALU.add)
-            rows4 = rows[:].rearrange("p (j h) e -> p j h e", h=2)
-            nc.vector.tensor_scalar(out=rows4[:, :, 1, :], in0=rows4[:, :, 1, :], scalar1=1.0, scalar2=None, op0=ALU.add)
-            nc.vector.tensor_copy(out=idx[:].rearrange("p j h e -> p (j h e)"), in_=rows[:].rearrange("p q e -> p (q e)"))
+                nc.vector.tensor_tensor(out=part[:, e, :, :], in0=step[:],
+                                        in1=gain[:, e, :].unsqueeze(2).to_broadcast([P, NS, NQ]), op=ALU.mult)
 
+        def window_rows():
+            total = const.tile([P, 2, NQ], F32)
+            nc.vector.tensor_reduce(out=total[:].rearrange("p e q -> p (e q)"), in_=part[:].rearrange("p e k q -> p e q k"),
+                                    axis=AX.X, op=ALU.add)
+            for e in range(2):
+                nc.vector.tensor_tensor(out=fl3[:, :, e], in0=fl3[:, :, e], in1=step[:, 1, :], op=ALU.mult)
+            nc.vector.scalar_tensor_tensor(out=idx[:].rearrange("p j h e -> p (j h) e"), in0=fl3, scalar=5.0,
+                                           in1=total[:].rearrange("p e q -> p q e"), op0=ALU.mult, op1=ALU.add)
 
-        with tc.tile_pool(name="wstage", bufs=1) as wstage:
-            w_sb = wstage.tile([P, NM, C], BF16)
-            nc.scalar.dma_start(out=seg_bf[:], in_=segments.rearrange("(j l) n s -> (l n) j s", l=2))
-            for mp in range(NM // 2):
-                nc.sync.dma_start(out=w_sb[:, 2 * mp:2 * mp + 2, :],
-                                  in_=w_lr.rearrange("(p m) k -> p m k", m=NM)[:, 2 * mp:2 * mp + 2, :])
-                if mp == 0:
-                    load_piece(0)
-            load_piece(1)
-            for i, v in enumerate((b_lr, g_lr, be_lr)):
-                nc.scalar.dma_start(out=vec_bf[i][:], in_=v.rearrange("(p m) -> p m", m=NM))
-            make_identity(nc, ident[:])
-            nc.gpsimd.iota(pid_i[:], pattern=[[0, 1]], base=0, channel_multiplier=1)
-            nc.gpsimd.memset(tab[:], 0.0)
-            gather_indices()
+        wstage = ctx.enter_context(tc.tile_pool(name="wstage", bufs=1))
+        w_sb = wstage.tile([P, NM, C], BF16)
+        nc.scalar.dma_start(out=seg_bf[:].rearrange("p j h e -> p j (h e)"), in_=segments.rearrange("(j l) n s -> (l n) j s", l=2))
+        for mp in range(NM // 2):
+            nc.sync.dma_start(out=w_sb[:, 2 * mp:2 * mp + 2, :],
+                              in_=w_lr.rearrange("(p m) k -> p m k", m=NM)[:, 2 * mp:2 * mp + 2, :])
+            if mp == 0:
+                load_piece(0)
+        load_piece(1)
+        for i, v in enumerate((b_lr, g_lr, be_lr)):
+            nc.gpsimd.dma_start(out=vec_bf[i][:], in_=v.rearrange("(p m) -> p m", m=NM))
+        for k in range(1, TAB):
+            used = ZERO if k == TAB - 1 else 2 * N_OK[k]
+            nc.vector.memset(tab[:, k - 1, :, :, used:P], 0.0)
 
-            w_words = w_sb[:].bitcast(F32).rearrange("p m (q u) -> p m q u", u=2)
-            w_grp = wstage.tile([P, NM, P, 4], BF16, align_bytes=64)
-            w_grp32 = w_grp[:].bitcast(F32)
-            for mp in range(NM // 2):
-                wt = tpsum.tile([P, 4, P], F32, tag="tp")
-                for i in range(2):
-                    for u in range(2):
-                        nc.tensor.transpose(wt[:, 2 * i + u, :], w_words[:, 2 * mp + i, :, u], ident[:])
-                nc.scalar.copy(out=w_grp32[:, 2 * mp, :, :], in_=wt[:, 0:2, :].rearrange("p u r -> p r u"))
-                nc.scalar.copy(out=w_grp32[:, 2 * mp + 1, :, :], in_=wt[:, 2:4, :].rearrange("p u r -> p r u"))
-                if mp == 0:
-                    quantise_piece(0)
-                if mp % 2 == 1:
-                    ms = slice(2 * mp - 2, 2 * mp + 2)
-                    nc.vector.quantize_mx(out=w_codes[:, ms, :].rearrange("p m c -> p (m c)").bitcast(FP8X4),
-                                          scales=w_scales[:, ms, :].rearrange("p m c -> p (m c)"),
-                                          in_=w_grp[:, ms, :, :].rearrange("p m c j -> p (m c j)"))
+        w_words = w_sb[:].bitcast(F32).rearrange("p m (q u) -> p m q u", u=2)
+        w_grp = wstage.tile([P, NM, P, 4], BF16, align_bytes=64)
+        w_grp32 = w_grp[:].bitcast(F32)
 
-        grp = const.tile([P, 32], F32)
-        nc.vector.tensor_reduce(out=grp[:], in_=ident[:].rearrange("p (q r) -> p q r", r=4), axis=AX.X, op=ALU.add)
-        bd = const.tile([P, 32, 4], F32)
-        nc.vector.tensor_scalar(out=bd[:], in0=grp[:].unsqueeze(2).to_broadcast([P, 32, 4]),
-                                scalar1=1.0 / 2048.0, scalar2=None, op0=ALU.mult)
-        bd2 = bd[:].rearrange("p q r -> p (q r)")
-        vec = const.tile([P, 3, NM], F32)
-        for i in range(3):
-            nc.vector.tensor_copy(out=vec[:, i, :], in_=vec_bf[i][:])
-        beta = vec[:, 0, :]
-        gamma = vec[:, 1, :]
-        shift0 = vec[:, 2, :]
-        beta2 = const.tile([P, NM], F32)
-        nc.vector.tensor_scalar(out=beta2[:], in0=beta, scalar1=2.0, scalar2=None, op0=ALU.mult)
-        bsq = const.tile([P, NM], F32)
-        nc.vector.tensor_tensor(out=bsq[:], in0=beta, in1=beta, op=ALU.mult)
+        def quantise_w(hb):
+            ms = slice(4 * hb, 4 * hb + 4)
+            nc.vector.quantize_mx(out=w_codes[:, ms, :].rearrange("p m c -> p (m c)").bitcast(FP8X4),
+                                  scales=w_scales[:, ms, :].rearrange("p m c -> p (m c)"),
+                                  in_=w_grp[:, ms, :, :].rearrange("p m c j -> p (m c j)"))
+
+        for mp in range(NM // 2):
+            wt = tpsum.tile([P, 4, P], F32, name="wt", tag="tp")
+            for i in range(2):
+                for u in range(2):
+                    nc.tensor.transpose(wt[:, 2 * i + u, :], w_words[:, 2 * mp + i, :, u], ident[:])
+            nc.scalar.copy(out=w_grp32[:, 2 * mp, :, :], in_=wt[:, 0:2, :].rearrange("p u r -> p r u"))
+            nc.scalar.copy(out=w_grp32[:, 2 * mp + 1, :, :], in_=wt[:, 2:4, :].rearrange("p u r -> p r u"))
+
         cc = const.tile([P, 2], F32)
-        nc.vector.tensor_reduce(out=cc[:, 0:1], in_=beta, axis=AX.X, op=ALU.add)
-        nc.vector.tensor_reduce(out=cc[:, 1:2], in_=bsq[:], axis=AX.X, op=ALU.add)
-        cc64 = const.tile([P, 2], F32)
-        nc.vector.tensor_scalar(out=cc64[:], in0=cc[:], scalar1=64.0, scalar2=None, op0=ALU.mult)
-        cg_ps = opsum.tile([P, 2], F32, tag="op")
-        nc.tensor.matmul(out=cg_ps[:], lhsT=bd2, rhs=cc64[:], start=True, stop=True)
         cg = const.tile([P, 2], F32)
-        nc.vector.tensor_copy(out=cg[:], in_=cg_ps[:])
+
+        def norm_constants():
+            bsq = const.tile([P, NM], F32)
+            nc.vector.tensor_tensor(out=bsq[:], in0=beta, in1=beta, op=ALU.mult)
+            nc.vector.tensor_reduce(out=cc[:, 0:1], in_=beta, axis=AX.X, op=ALU.add)
+            nc.vector.tensor_reduce(out=cc[:, 1:2], in_=bsq[:], axis=AX.X, op=ALU.add)
 
         fpool = ctx.enter_context(tc.tile_pool(name="fpool", bufs=2))
-        late = ctx.enter_context(tc.tile_pool(name="late", bufs=5))
+        late = ctx.enter_context(tc.tile_pool(name="late", bufs=LATE))
         rpool = ctx.enter_context(tc.tile_pool(name="rpool", bufs=2))
         gpool = ctx.enter_context(tc.tile_pool(name="gpool", bufs=2))
         opool = ctx.enter_context(tc.tile_pool(name="opool", bufs=2))
 
         slots = [out_0, out_1]
-        slot_store = [o[0:SLOT_B].rearrange("b (x c) t -> (b x) (c t)", c=16).rearrange("(r k) w -> r k w", k=TAB)
+        slot_store = [o[0:SLOT_B].rearrange("(h b) (x c) t -> h (b x) (c t)", h=2, c=8).rearrange("h (r k) w -> r h k w", k=TAB)
                       for o in slots]
         slot_rows = [o[0:SLOT_B].rearrange("b (x c) t -> (b x) (c t)", c=8) for o in slots]
 
@@ -215,81 +199,108 @@ def tile_coarsepyramid_pa_kernel(tc, feature, segments, w_lr, b_lr, g_lr, be_lr,
                                     rhs=x_codes[:, cols].bitcast(FP8X4), rhs_scale=x_scales[:, cols],
                                     start=True, stop=True)
 
-        def sums_mx(pos, hb):
+        def group_of(pos):
+            for q in range(len(pieces)):
+                p0 = first_use(q)
+                if p0 <= pos < p0 + pieces[q][1] // 2:
+                    return q, 2 * (pos - p0)
+
+        def squares(pos):
             if pos >= NCH:
                 return
-            ysum = ypsum.tile([P, 4, P], F32, name="ysum%d" % hb, tag="ysum%d" % hb)
-            mx_passes(ysum, pos, hb)
-            live[("ysum", hb)] = ysum
+            q, bi = group_of(pos)
+            if bi == 0:
+                live[("terms", q)] = small.tile([P, NM + 2, 8], F32, name="terms", tag="terms")
+            terms = live[("terms", q)]
+            ys = []
+            for hb in range(2):
+                y = ypsum.tile([P, 4, P], F32, name="y%d" % hb, tag="y%d" % hb)
+                mx_passes(y, pos, hb)
+                ys.append(y)
+            for hb in range(2):
+                junk = small.tile([P, 4, T], F32, name="junk", tag="junk")
+                for l in range(2):
+                    nc.scalar.activation(out=junk[:], in_=ys[hb][:, :, T * l:T * l + T], func=ACT.Square,
+                                         accum_out=terms[:, NM + hb, bi + l:bi + l + 1])
 
-        def sums(pos, hb):
-            if pos >= NCH:
-                return
-            g, e = pos // 2, pos % 2
-            if e == 0 and hb == 0:
-                live[("s1", g)] = small.tile([P, 2, NM, 2], F32, name="s1", tag="s1")
-                live[("acc", g)] = small.tile([P, 2, 2, 2], F32, name="acc", tag="acc")
-            s1 = live[("s1", g)]
-            acc = live[("acc", g)]
-            ysum = live[("ysum", hb)]
-            junk = small.tile([P, 4, T], F32)
-            nc.vector.tensor_reduce(out=s1[:, e, 4 * hb:4 * hb + 4, :].rearrange("p m l -> p (m l)"),
-                                    in_=ysum[:].rearrange("p m (l t) -> p (m l) t", l=2), axis=AX.X, op=ALU.add)
-            for l in range(2):
-                nc.scalar.activation(out=junk[:], in_=ysum[:, :, T * l:T * l + T], func=ACT.Square,
-                                     accum_out=acc[:, e, hb, l:l + 1])
+        def reorder_codes(q):
+            b0, nb = pieces[q]
+            n = T * nb
+            xt = stage.tile([P, 8 * T], U32, align_bytes=64, name="xt", tag="xt")
+            xts = stage.tile([P, 8 * T], U8, align_bytes=64, name="xts", tag="xts")
+            nc.vector.tensor_copy(out=xt[:, 0:n].bitcast(I32).rearrange("p (t b) -> p t b", b=nb),
+                                  in_=x_codes[:, T * b0:T * b0 + n].bitcast(I32).rearrange("p (b t) -> p t b", b=nb))
+            nc.vector.tensor_copy(out=xts[:, 0:n].rearrange("p (t b) -> p b t", b=nb),
+                                  in_=x_scales[:, T * b0:T * b0 + n].rearrange("p (b t) -> p b t", b=nb))
+            live[("xt", q)] = (xt, xts)
 
-        def chain_a(g):
-            if g >= NCH // 2:
-                return
-            s1 = live[("s1", g)]
-            acc = live[("acc", g)]
-            cross = small.tile([P, 2, NM, 2], F32)
-            nc.vector.tensor_tensor(out=cross[:], in0=s1[:],
-                                    in1=beta2[:].unsqueeze(1).unsqueeze(3).to_broadcast([P, 2, NM, 2]), op=ALU.mult)
-            rs = small.tile([P, 2, 2, 2], F32)
-            nc.vector.tensor_reduce(out=rs[:, 0, :, :], in_=s1[:].rearrange("p e m l -> p e l m"), axis=AX.X, op=ALU.add)
-            nc.vector.tensor_reduce(out=rs[:, 1, :, :], in_=cross[:].rearrange("p e m l -> p e l m"), axis=AX.X, op=ALU.add)
-            nc.vector.tensor_tensor(out=rs[:, 1, :, :], in0=rs[:, 1, :, :], in1=acc[:, :, 0, :], op=ALU.add)
-            nc.vector.tensor_tensor(out=rs[:, 1, :, :], in0=rs[:, 1, :, :], in1=acc[:, :, 1, :], op=ALU.add)
-            st = opsum.tile([P, 2, 4], F32, tag="op")
-            nc.tensor.matmul(out=st[:].rearrange("p s x -> p (s x)"), lhsT=bd2, rhs=rs[:].rearrange("p s e l -> p (s e l)"),
-                             start=True, stop=True)
-            live[("st", g)] = st
+        def piece_sums(q):
+            nb = pieces[q][1]
+            n = T * nb
+            xt, xts = live[("xt", q)]
+            s1 = small.tile([P, NM, 8], F32, name="s1", tag="s1")
+            for hb in range(2):
+                y = ypsum.tile([P, 4, P], F32, name="ysum%d" % hb, tag="y%d" % hb)
+                for i in range(4):
+                    m = 4 * hb + i
+                    for u in range(n // P):
+                        cols = slice(P * u, P * u + P)
+                        nc.tensor.matmul_mx(out=y[:, i, :], lhsT=w_codes[:, m, :].bitcast(FP8X4), lhsT_scale=w_scales[:, m, :],
+                                            rhs=xt[:, cols].bitcast(FP8X4), rhs_scale=xts[:, cols],
+                                            start=u == 0, stop=u == n // P - 1)
+                nc.vector.tensor_reduce(out=s1[:, 4 * hb:4 * hb + 4, 0:nb],
+                                        in_=y[:].rearrange("p m (t b) -> p m b t", b=nb), axis=AX.X, op=ALU.add)
+            live[("s1", q)] = s1
 
-        def chain_b(g):
-            if g >= NCH // 2:
-                return
-            st = live[("st", g)]
-            mv = small.tile([P, 2, 4], F32)
-            nc.vector.tensor_tensor(out=mv[:], in0=st[:], in1=cg[:].unsqueeze(2).to_broadcast([P, 2, 4]), op=ALU.add)
-            var = small.tile([P, 4], F32)
-            nc.vector.tensor_tensor(out=var[:], in0=mv[:, 0, :], in1=mv[:, 0, :], op=ALU.mult)
-            nc.vector.tensor_tensor(out=var[:], in0=mv[:, 1, :], in1=var[:], op=ALU.subtract)
-            nc.vector.tensor_scalar(out=var[:], in0=var[:], scalar1=EPS, scalar2=None, op0=ALU.add)
-            std = small.tile([P, 4], F32)
-            nc.scalar.activation(out=std[:], in_=var[:], func=ACT.Sqrt)
-            live[("mv", g)] = mv
-            live[("std", g)] = std
+        def chain_a(q):
+            nb = pieces[q][1]
+            s1 = live[("s1", q)]
+            terms = live[("terms", q)]
+            rs = small.tile([P, 16], F32, name="rs", tag="rs")
+            if q == 0:
+                cg_ps = opsum.tile([P, 2], F32, name="cg_ps", tag="op")
+                nc.tensor.matmul(out=cg_ps[:], lhsT=ones4[:], rhs=cc[:], start=True, stop=True)
+                nc.vector.tensor_scalar(out=cg[:], in0=cg_ps[:], scalar1=64.0 / 2048.0, scalar2=None, op0=ALU.mult)
+            nc.vector.scalar_tensor_tensor(out=terms[:, 0:NM, 0:nb], in0=s1[:, :, 0:nb], scalar=2.0,
+                                           in1=beta.unsqueeze(2).to_broadcast([P, NM, nb]), op0=ALU.mult, op1=ALU.mult)
+            nc.vector.tensor_reduce(out=rs[:, 0:nb], in_=s1[:, :, 0:nb].rearrange("p m b -> p b m"), axis=AX.X, op=ALU.add)
+            if q == 0:
+                window_steps()
+            nc.vector.tensor_reduce(out=rs[:, nb:2 * nb], in_=terms[:, :, 0:nb].rearrange("p m b -> p b m"), axis=AX.X, op=ALU.add)
+            st = opsum.tile([P, 16], F32, name="st", tag="op")
+            nc.tensor.matmul(out=st[:, 0:2 * nb], lhsT=ones4[:], rhs=rs[:, 0:2 * nb], start=True, stop=True)
+            live[("st", q)] = st
 
-        def chain_c(g):
-            if g >= NCH // 2:
-                return
-            mv = live[("mv", g)]
-            rstd = small.tile([P, 2, 2], F32)
-            nc.vector.reciprocal(out=rstd[:].rearrange("p e l -> p (e l)"), in_=live[("std", g)][:])
-            full = [P, 2, NM, 2]
-            sc = small.tile(full, F32)
-            nc.vector.tensor_tensor(out=sc[:], in0=gamma.unsqueeze(1).unsqueeze(3).to_broadcast(full),
-                                    in1=rstd[:].unsqueeze(2).to_broadcast(full), op=ALU.mult)
-            sh = small.tile(full, F32)
-            nc.vector.tensor_tensor(out=sh[:], in0=beta.unsqueeze(1).unsqueeze(3).to_broadcast(full),
-                                    in1=mv[:, 0, :].rearrange("p (e l) -> p e l", e=2).unsqueeze(2).to_broadcast(full),
-                                    op=ALU.subtract)
-            nc.vector.tensor_tensor(out=sh[:], in0=sh[:], in1=sc[:], op=ALU.mult)
-            nc.vector.tensor_tensor(out=sh[:], in0=sh[:], in1=shift0.unsqueeze(1).unsqueeze(3).to_broadcast(full), op=ALU.add)
-            live[("sc", g)] = sc
-            live[("sh", g)] = sh
+        def chain_b(q):
+            nb = pieces[q][1]
+            st = live[("st", q)]
+            mv = small.tile([P, 2, 8], F32, name="mv", tag="mv")
+            nc.vector.scalar_tensor_tensor(out=mv[:, :, 0:nb], in0=st[:, 0:2 * nb].rearrange("p (s b) -> p s b", s=2), scalar=1.0 / 2048.0,
+                                           in1=cg[:].unsqueeze(2).to_broadcast([P, 2, nb]), op0=ALU.mult, op1=ALU.add)
+            var = small.tile([P, 8], F32, name="var", tag="var")
+            nc.vector.tensor_tensor(out=var[:, 0:nb], in0=mv[:, 0, 0:nb], in1=mv[:, 0, 0:nb], op=ALU.mult)
+            nc.vector.scalar_tensor_tensor(out=var[:, 0:nb], in0=mv[:, 1, 0:nb], scalar=EPS, in1=var[:, 0:nb], op0=ALU.add, op1=ALU.subtract)
+            std = small.tile([P, 8], F32, name="std", tag="std")
+            nc.scalar.activation(out=std[:, 0:nb], in_=var[:, 0:nb], func=ACT.Sqrt)
+            live[("mv", q)] = mv
+            live[("std", q)] = std
+
+        def chain_c(q):
+            nb = pieces[q][1]
+            mv = live[("mv", q)]
+            full = [P, NM, nb]
+            sh = small.tile([P, NM, 8], F32, name="sh", tag="sh")
+            nc.vector.tensor_tensor(out=sh[:, :, 0:nb], in0=beta.unsqueeze(2).to_broadcast(full),
+                                    in1=mv[:, 0, 0:nb].unsqueeze(1).to_broadcast(full), op=ALU.subtract)
+            rstd = small.tile([P, 8], F32, name="rstd", tag="rstd")
+            nc.vector.reciprocal(out=rstd[:, 0:nb], in_=live[("std", q)][:, 0:nb])
+            sc = small.tile([P, NM, 8], F32, name="sc", tag="sc")
+            nc.vector.tensor_tensor(out=sc[:, :, 0:nb], in0=gamma.unsqueeze(2).to_broadcast(full),
+                                    in1=rstd[:, 0:nb].unsqueeze(1).to_broadcast(full), op=ALU.mult)
+            nc.vector.tensor_tensor(out=sh[:, :, 0:nb], in0=sh[:, :, 0:nb], in1=sc[:, :, 0:nb], op=ALU.mult)
+            nc.vector.tensor_tensor(out=sh[:, :, 0:nb], in0=sh[:, :, 0:nb], in1=shift0.unsqueeze(2).to_broadcast(full), op=ALU.add)
+            live[("sc", q)] = sc
+            live[("sh", q)] = sh
 
         def main_mx(pos):
             ys = []
@@ -298,19 +309,21 @@ def tile_coarsepyramid_pa_kernel(tc, feature, segments, w_lr, b_lr, g_lr, be_lr,
                 mx_passes(y, pos, hb)
                 ys.append(y)
             live[("y", pos)] = ys
-            live[("f", pos)] = fpool.tile([P, NM, P], F32, name="f", tag="f")
 
         def apply_norm(pos, hb):
+            if hb == 0:
+                live[("f", pos)] = fpool.tile([P, 2, 4, P], F32, name="f", tag="f")
             f = live[("f", pos)]
-            y = live[("y", pos)][hb]
-            sc = live[("sc", pos // 2)]
-            sh = live[("sh", pos // 2)]
-            e = pos % 2
+            ys = live[("y", pos)]
+            q, bi = group_of(pos)
+            sc = live[("sc", q)]
+            sh = live[("sh", q)]
             for i in range(4):
                 m = 4 * hb + i
                 for l in range(2):
-                    nc.scalar.activation(out=f[:, m, T * l:T * l + T], in_=y[:, i, T * l:T * l + T],
-                                         func=ACT.Relu, bias=sh[:, e, m, l:l + 1], scale=sc[:, e, m, l:l + 1])
+                    b = bi + l
+                    nc.scalar.activation(out=f[:, m % 2, m // 2, T * l:T * l + T], in_=ys[hb][:, i, T * l:T * l + T],
+                                         func=ACT.Relu, bias=sh[:, m, b:b + 1], scale=sc[:, m, b:b + 1])
 
         def send(x, dst, src):
             if held[x] is None:
@@ -323,85 +336,91 @@ def tile_coarsepyramid_pa_kernel(tc, feature, segments, w_lr, b_lr, g_lr, be_lr,
                 nc.sync.dma_start(out=dst, in_=src)
             held[x] = None
 
+        def copy_feat(pos, l):
+            if l == 0:
+                if order[pos] < LATE:
+                    live[("f2", pos)] = late.tile([P, 2, NM, T], F32, name="f2_late", tag="f2_late")
+                else:
+                    live[("f2", pos)] = opool.tile([P, 2, NM, T], F32, name="f2", tag="f2")
+            nc.scalar.copy(out=live[("f2", pos)][:, l, :, :].rearrange("p (j mm) t -> p j mm t", mm=2),
+                           in_=live[("f", pos)][:, :, :, T * l:T * l + T].rearrange("p mm j t -> p j mm t"))
+
         def store_feat(pos):
             j = order[pos]
-            is_late = j < SLOT_B // 2
-            f = live[("f", pos)]
-            if is_late:
-                f2 = late.tile([P, 2, NM, T], F32, name="f2_late", tag="f2_late")
-            else:
-                f2 = opool.tile([P, 2, NM, T], F32, name="f2", tag="f2")
-            nc.scalar.copy(out=f2[:], in_=f[:].rearrange("p m (l t) -> p l m t", l=2))
             dst = out_0[2 * j:2 * j + 2].rearrange("l (p m) t -> p l (m t)", m=NM)
-            if is_late:
-                send(0, dst, f2[:].rearrange("p l m t -> p l (m t)"))
+            src = live[("f2", pos)][:].rearrange("p l m t -> p l (m t)")
+            if j < LATE:
+                send(0, dst, src)
             else:
-                nc.sync.dma_start(out=dst, in_=f2[:].rearrange("p l m t -> p l (m t)"))
+                nc.sync.dma_start(out=dst, in_=src)
 
-        def view(k):
+        def view(k, mm):
             if k == 5:
-                cols = tab[:, 3, :, TOP:TOP + 2 * N_OK[5]]
+                cols = tab[:, 3, mm, :, TOP:TOP + 2 * N_OK[5]]
             else:
-                cols = tab[:, k - 1, :, 0:2 * N_OK[k]]
-            return cols.rearrange("p m (l t) -> p m l t", l=2)
+                cols = tab[:, k - 1, mm, :, 0:2 * N_OK[k]]
+            return cols.rearrange("p j (l t) -> p j l t", l=2)
+
+        def window(out, in_, shift, n):
+            nc.vector.tensor_tensor(out=out, in0=in_[:, :, :, 0:n], in1=in_[:, :, :, shift:shift + n], op=ALU.max)
+
+        def pairs_up(pos):
+            for mm in range(2):
+                window(pairs[:, mm, :, :].rearrange("p j (l t) -> p j l t", l=2),
+                       live[("f", pos)][:, mm, :, :].rearrange("p j (l t) -> p j l t", l=2), 1, T - 1)
 
         def level_up(pos, k):
-            n_ok = N_OK[k + 1]
-            if k == 0:
-                f = live[("f", pos)][:].rearrange("p m (l t) -> p m l t", l=2)
-                two = pairs[:].rearrange("p m (l t) -> p m l t", l=2)
-                nc.vector.tensor_tensor(out=two, in0=f[:, :, :, 0:T - 1], in1=f[:, :, :, 1:T], op=ALU.max)
-                prev, s = two, 1
-            else:
-                prev, s = view(k), SIZES[k]
-            nc.vector.tensor_tensor(out=view(k + 1), in0=prev[:, :, :, 0:n_ok], in1=prev[:, :, :, s:s + n_ok], op=ALU.max)
+            for mm in range(2):
+                if k == 0:
+                    window(view(1, mm), pairs[:, mm, :, :].rearrange("p j (l t) -> p j l t", l=2), 1, N_OK[1])
+                else:
+                    window(view(k + 1, mm), view(k, mm), SIZES[k], N_OK[k + 1])
 
         def rows_out(pos, k):
-            f = live[("f", pos)]
-            if k == 0:
-                live[("r", pos)] = rpool.tile([P, TAB, 2, NM, 64], F32, name="r", tag="r")
-            r = live[("r", pos)]
-            for hb in range(2):
-                tp = tpsum.tile([P, 4, P], F32, tag="tp")
-                for i in range(4):
-                    m = 4 * hb + i
-                    src = f[:, m, :] if k == 0 else tab[:, k - 1, m, :]
-                    nc.tensor.transpose(tp[:, i, :], src, ident[:])
-                dst = r[:, k, :, 4 * hb:4 * hb + 4, :]
-                rows = tp[:].rearrange("p m (h q) -> p h m q", h=2)
+            u, first = k // 2, k % 2 == 0
+            if first:
+                n = 2 if k < TAB - 1 else 1
+                live[("r", pos, u)] = rpool.tile([P, 2, n, 2, 4, 64], F32, name="r%d" % u, tag="r%d" % u)
+            r = live[("r", pos, u)]
+            for mm in range(2):
+                tp = tpsum.tile([P, 4, P], F32, name="tp", tag="tp")
+                for j in range(4):
+                    src = live[("f", pos)][:, mm, j, :] if k == 0 else tab[:, k - 1, mm, j, :]
+                    nc.tensor.transpose(tp[:, j, :], src, ident[:])
+                dst = r[:, :, k % 2, mm, :, :]
+                rows = tp[:].rearrange("p j (h q) -> p h j q", h=2)
                 if k == TAB - 1:
                     nc.vector.tensor_copy(out=dst, in_=rows)
                 else:
                     nc.scalar.copy(out=dst, in_=rows)
-            if k != 0 and k != 2:
-                first = k - 1 if k < TAB - 1 else k
-                nc.sync.dma_start(out=slot_store[pos % 2][:, first:k + 1, :],
-                                  in_=r[:, first:k + 1, :, :, :].rearrange("p k h m q -> p k (h m q)"))
+
+        def store_rows(pos, u, h):
+            r = live[("r", pos, u)]
+            nc.sync.dma_start(out=slot_store[pos % 2][:, h, 2 * u:min(2 * u + 2, TAB), :],
+                              in_=r[:, h, :, :, :, :].rearrange("p k mm j q -> p k (mm j q)"))
 
         def gathers(pos):
             j = order[pos]
-            got = []
-            for h in range(2):
-                ga = gpool.tile([P, C], F32, name="ga%d" % h, tag="ga%d" % h, bufs=3)
-                gb = gpool.tile([P, C], F32, name="gb%d" % h, tag="gb%d" % h, bufs=3)
-                nc.gpsimd.indirect_dma_start(out=ga[:], out_offset=None, in_=slot_rows[pos % 2],
-                                             in_offset=bass.IndirectOffsetOnAxis(ap=idx[:, j, h, 0:1], axis=0))
-                nc.gpsimd.indirect_dma_start(out=gb[:], out_offset=None, in_=slot_rows[pos % 2],
-                                             in_offset=bass.IndirectOffsetOnAxis(ap=idx[:, j, h, 1:2], axis=0))
-                got.append((ga, gb))
+            got = {}
+            for h in (1, 0):
+                rows = slot_rows[pos % 2][0:128 * TAB * (h + 1), :]
+                for e in range(2):
+                    g = gpool.tile([P, C], F32, name="g%d%d" % (h, e), tag="g%d%d" % (h, e), bufs=3)
+                    nc.gpsimd.indirect_dma_start(out=g[:], out_offset=None, in_=rows,
+                                                 in_offset=bass.IndirectOffsetOnAxis(ap=idx[:, j, h, e:e + 1], axis=0))
+                    got[(h, e)] = g
             live[("g", pos)] = got
 
-        def window_max(pos):
-            gc = gpool.tile([P, NM, 2, 64], F32)
-            for h in range(2):
-                ga, gb = live[("g", pos)][h]
-                nc.vector.tensor_tensor(out=gc[:, :, h, :], in0=ga[:].rearrange("p (m q) -> p m q", m=NM),
-                                        in1=gb[:].rearrange("p (m q) -> p m q", m=NM), op=ALU.max)
-            live[("gc", pos)] = gc
+        def window_max(pos, h):
+            if h == 1:
+                live[("gc", pos)] = gpool.tile([P, NM, 2, 64], F32, name="gc", tag="gc")
+            got = live[("g", pos)]
+            nc.vector.tensor_tensor(out=live[("gc", pos)][:, :, h, :], in0=got[(h, 0)][:].rearrange("p (m q) -> p m q", m=NM),
+                                    in1=got[(h, 1)][:].rearrange("p (m q) -> p m q", m=NM), op=ALU.max)
 
         def pooled_out(pos, hb):
             j = order[pos]
-            is_late = j < SLOT_B // 2
+            is_late = j < LATE
             gc = live[("gc", pos)]
             if hb == 0:
                 if is_late:
@@ -409,9 +428,9 @@ def tile_coarsepyramid_pa_kernel(tc, feature, segments, w_lr, b_lr, g_lr, be_lr,
                 else:
                     live[("o", pos)] = opool.tile([P, 2, NM, T], F32, name="o", tag="o")
             o = live[("o", pos)]
-            op = opsum.tile([P, 4, P], F32, tag="op")
+            op = opsum.tile([P, 4, P], F32, name="op", tag="op")
             for i in range(4):
-                nc.tensor.transpose(op[:, i, :], gc[:, 4 * hb + i, :, :].rearrange("p h q -> p (h q)"), ident[:])
+                nc.tensor.transpose(op[:, i, :], gc[:, 4 * (i % 2) + 2 * hb + i // 2, :, :].rearrange("p h q -> p (h q)"), ident[:])
             nc.scalar.copy(out=o[:, :, 4 * hb:4 * hb + 4, :], in_=op[:].rearrange("p m (l n) -> p l m n", l=2))
             if hb == 1:
                 dst = out_1[2 * j:2 * j + 2].rearrange("l (p m) n -> p l (m n)", m=NM)
@@ -420,73 +439,100 @@ def tile_coarsepyramid_pa_kernel(tc, feature, segments, w_lr, b_lr, g_lr, be_lr,
                 else:
                     nc.sync.dma_start(out=dst, in_=o[:].rearrange("p l m n -> p l (m n)"))
 
-        for pos in range(2):
-            for hb in range(2):
-                sums_mx(pos, hb)
-                sums(pos, hb)
+        def group_all(q):
+            for b in range(0, pieces[q][1], 2):
+                group_piece(q, b)
+
+        def one_round(a):
+            c = a - 1
+            w = c - 3
+            first = a < NCH
+            second = 0 <= c < NCH
+            third = 0 <= w < NCH
+            starts = [q for q in range(1, len(pieces)) if first_use(q) == a]
+            if second:
+                rows_out(c, 0)
+                pairs_up(c)
+            if a >= 4:
+                squares(a + 3)
+            for q in range(1, len(pieces)):
+                if a == (first_use(q) - 4 if q > 3 else q):
+                    group_all(q)
+            if second:
+                level_up(c, 0)
+                rows_out(c, 1)
+                store_rows(c, 0, 1)
+                store_rows(c, 0, 0)
+                copy_feat(c, 0)
+                copy_feat(c, 1)
+                store_feat(c)
+            for q in starts:
+                piece_sums(q)
+                chain_a(q)
+            if third:
+                window_max(w, 1)
+            if second:
+                level_up(c, 1)
+                rows_out(c, 2)
+            for q in range(1, len(pieces)):
+                if a == (first_use(q) - 4 if q > 3 else q):
+                    quantise_piece(q)
+                if a == first_use(q) - 1:
+                    reorder_codes(q)
+            for q in starts:
+                chain_b(q)
+            if third:
+                window_max(w, 0)
+                if w >= NCH - 2:
+                    give_up_slot(w % 2)
+            if second:
+                level_up(c, 2)
+            for q in starts:
+                chain_c(q)
+            if second:
+                rows_out(c, 3)
+                store_rows(c, 1, 1)
+                store_rows(c, 1, 0)
+            if first:
+                main_mx(a)
+                apply_norm(a, 0)
+                apply_norm(a, 1)
+            if second:
+                level_up(c, 3)
+                level_up(c, 4)
+                rows_out(c, 4)
+                store_rows(c, 2, 1)
+                store_rows(c, 2, 0)
+                gathers(c)
+            if third:
+                pooled_out(w, 0)
+                pooled_out(w, 1)
+            for q in range(1, len(pieces)):
+                p0 = first_use(q)
+                if a == (p0 - 7 if q > 3 else max(q - 2, 0)) and q > 1:
+                    load_piece(q)
+            if a in (1, 2):
+                squares(2 * a)
+                squares(2 * a + 1)
+            if a == 3:
+                squares(6)
+
+        step_constants()
+        warm = const.tile([P, 1], F32)
+        nc.scalar.activation(out=warm[:], in_=thr[:, 1:2], func=ACT.Sqrt)
+        window_ends()
+        group_all(0)
+        quantise_piece(0)
+        norm_constants()
+        reorder_codes(0)
+        quantise_w(0)
+        quantise_w(1)
+        piece_sums(0)
+        squares(0)
+        squares(1)
         chain_a(0)
         chain_b(0)
         chain_c(0)
+        window_rows()
         for a in range(NCH + 4):
-            first = a < NCH
-            second = 0 <= a - 1 < NCH
-            third = 0 <= a - 3 < NCH
-            fourth = 0 <= a - 4 < NCH
-            g_next = (a + 1) // 2 if a % 2 == 1 else NCH
-            for q in range(2, len(pieces)):
-                if first_use(q) - 6 == a:
-                    load_piece(q)
-            if fourth:
-                pooled_out(a - 4, 0)
-            if second:
-                rows_out(a - 1, 0)
-                level_up(a - 1, 0)
-            if first:
-                main_mx(a)
-            if a == 1:
-                quantise_piece(1)
-            if second:
-                level_up(a - 1, 1)
-                rows_out(a - 1, 1)
-            if a == 0:
-                apply_norm(a, 0)
-                apply_norm(a, 1)
-                store_feat(a)
-            if a > 0:
-                sums_mx(a + 3, 0)
-                sums_mx(a + 3, 1)
-            if second:
-                level_up(a - 1, 2)
-                rows_out(a - 1, 2)
-                level_up(a - 1, 3)
-                rows_out(a - 1, 3)
-                level_up(a - 1, 4)
-                rows_out(a - 1, 4)
-                gathers(a - 1)
-            if a == 1:
-                sums(a + 3, 0)
-                sums(a + 3, 1)
-                for pos in (2, 3):
-                    for hb in range(2):
-                        sums_mx(pos, hb)
-                        sums(pos, hb)
-            chain_a(g_next)
-            if first and a > 0:
-                apply_norm(a, 0)
-                apply_norm(a, 1)
-                store_feat(a)
-            if a > 1:
-                sums(a + 3, 0)
-            chain_b(g_next)
-            if third:
-                window_max(a - 3)
-                if a - 3 >= NCH - 2:
-                    give_up_slot((a - 3) % 2)
-            if fourth:
-                pooled_out(a - 4, 1)
-            if a > 1:
-                sums(a + 3, 1)
-            chain_c(g_next)
-            for q in range(2, len(pieces)):
-                if first_use(q) - 4 == a:
-                    quantise_piece(q)
+            one_round(a)

@@ -37,11 +37,12 @@ def tile_coarsepyramid_pa_kernel(tc, feature, segments, w_lr, b_lr, g_lr, be_lr,
         small = ctx.enter_context(tc.tile_pool(name="small", bufs=3))
         stage = ctx.enter_context(tc.tile_pool(name="stage", bufs=2))
         ypsum = ctx.enter_context(tc.psum_pool(name="ypsum", bufs=1))
-        tpsum = ctx.enter_context(tc.psum_pool(name="tpsum", bufs=4))
+        tpsum = ctx.enter_context(tc.psum_pool(name="tpsum", bufs=3))
         opsum = ctx.enter_context(tc.psum_pool(name="opsum", bufs=2))
+        spsum = ctx.enter_context(tc.psum_pool(name="spsum", bufs=1))
 
         order = list(range(LATE, NCH)) + list(range(LATE))
-        live = {}
+        live = {"steps": []}
         held = {0: [], 1: []}
 
         pieces = [(10, 4), (14, 4), (18, 4), (22, 8), (30, 8), (38, 8), (46, 2), (0, 8), (8, 2)]
@@ -53,7 +54,7 @@ def tile_coarsepyramid_pa_kernel(tc, feature, segments, w_lr, b_lr, g_lr, be_lr,
 
         def load_piece(q):
             b0, nb = pieces[q]
-            raw = stage.tile([P, 8, 4, T], BF16, name="raw", tag="raw")
+            raw = stage.tile([P, 8, 4, T], BF16, name="raw", tag="raw", bufs=3)
             nc.sync.dma_start(out=raw[:, 0:nb, :, :].rearrange("p b j t -> p b (j t)"),
                               in_=feature[b0:b0 + nb].rearrange("b (p j) t -> p b (j t)", j=4))
             live[("raw", q)] = raw
@@ -84,32 +85,39 @@ def tile_coarsepyramid_pa_kernel(tc, feature, segments, w_lr, b_lr, g_lr, be_lr,
         ones4 = const.tile([P, P], F32)
         tab = const.tile([P, TAB - 1, 2, 4, P], F32)
         pairs = const.tile([P, 2, 4, 2 * (T - 1)], F32)
-        STEPS = [-1000.0, 0.0] + [float(w - 1) for w in SIZES[1:]]
+        STEPS = [-1000.0] + [float(w - 1) for w in SIZES[1:]]
         NS = len(STEPS)
         thr = const.tile([P, NS], F32)
         gain = const.tile([P, 2, NS], F32)
+        pid = const.tile([P, 1], I32)
+        zrow = const.tile([P, 2], F32)
         idx = const.tile([P, NCH, 2, 2], I32)
 
+        nc.gpsimd.iota(pid[:], pattern=[[0, 1]], base=0, channel_multiplier=1)
         make_identity(nc, ident[:])
         make_block_diagonal(nc, ones4[:], 4)
-        ctx.enter_context(tc.manual_schedule())
 
         def step_constants():
             for k in range(NS):
                 nc.vector.memset(thr[:, k:k + 1], STEPS[k])
             for l in range(2):
                 for e in range(2):
-                    at = [5.0 * (ZERO + 4 * l + e) + TAB - 1]
+                    at = []
                     for k in range(LEV):
                         row = l * N_OK[k] + (TOP if k == 5 else 0) - e * (SIZES[k] - 1)
-                        at.append(5.0 * row + min(k, TAB - 1))
+                        at.append(10.0 * row + 2.0 * min(k, TAB - 1))
                     for k in range(NS):
                         nc.vector.memset(gain[T * l:P, e, k:k + 1], at[k] - (at[k - 1] if k > 0 else 0.0))
+            low = const.tile([P, 1], I32)
+            nc.vector.tensor_single_scalar(out=low[:], in_=pid[:], scalar=15, op=ALU.bitwise_and)
+            for i in range(2):
+                s = 1.0 - 2.0 * i
+                nc.vector.tensor_scalar(out=zrow[:, i:i + 1], in0=low[:], scalar1=10.0 * s, scalar2=(20.0 * N_OK[3] + 6.0) * s, op0=ALU.mult, op1=ALU.add)
 
         NQ = NCH * 2
-        fl = const.tile([P, NCH, 2, 2], F32)
-        fl3 = fl[:].rearrange("p j h e -> p (j h) e")
+        fl = const.tile([P, NQ, 2], F32)
         ln = const.tile([P, NQ], F32)
+        wanted = const.tile([P, NQ, 2], F32)
         step = const.tile([P, NS, NQ], F32)
         part = const.tile([P, 2, NS, NQ], F32)
 
@@ -117,10 +125,10 @@ def tile_coarsepyramid_pa_kernel(tc, feature, segments, w_lr, b_lr, g_lr, be_lr,
             whole = const.tile([P, NQ, 2], I32)
             nc.vector.tensor_scalar(out=whole[:].rearrange("p q e -> p (q e)"), in0=seg_bf[:].rearrange("p j h e -> p (j h e)"),
                                     scalar1=0.0, scalar2=-0.498, op0=ALU.max, op1=ALU.add)
-            for h in range(2):
-                nc.vector.tensor_scalar(out=fl[:, :, h, :], in0=whole[:].rearrange("p (j h) e -> p j h e", h=2)[:, :, h, :],
-                                        scalar1=float(T - 1), scalar2=128.0 * h, op0=ALU.min, op1=ALU.add)
-            nc.vector.tensor_tensor(out=ln[:], in0=fl3[:, :, 1], in1=fl3[:, :, 0], op=ALU.subtract)
+            nc.vector.tensor_scalar(out=fl[:].rearrange("p q e -> p (q e)"), in0=whole[:].rearrange("p q e -> p (q e)"),
+                                    scalar1=float(T - 1), scalar2=None, op0=ALU.min)
+            nc.vector.tensor_tensor(out=ln[:], in0=fl[:, :, 1], in1=fl[:, :, 0], op=ALU.subtract)
+            nc.vector.tensor_scalar(out=wanted[:, :, 0], in0=ln[:], scalar1=0.0, scalar2=None, op0=ALU.is_ge)
 
         def window_steps():
             nc.vector.tensor_tensor(out=step[:], in0=ln[:].unsqueeze(1).to_broadcast([P, NS, NQ]),
@@ -133,10 +141,14 @@ def tile_coarsepyramid_pa_kernel(tc, feature, segments, w_lr, b_lr, g_lr, be_lr,
             total = const.tile([P, 2, NQ], F32)
             nc.vector.tensor_reduce(out=total[:].rearrange("p e q -> p (e q)"), in_=part[:].rearrange("p e k q -> p e q k"),
                                     axis=AX.X, op=ALU.add)
-            for e in range(2):
-                nc.vector.tensor_tensor(out=fl3[:, :, e], in0=fl3[:, :, e], in1=step[:, 1, :], op=ALU.mult)
-            nc.vector.scalar_tensor_tensor(out=idx[:].rearrange("p j h e -> p (j h) e"), in0=fl3, scalar=5.0,
-                                           in1=total[:].rearrange("p e q -> p q e"), op0=ALU.mult, op1=ALU.add)
+            size = const.tile([P, NQ], F32)
+            nc.vector.tensor_tensor(out=size[:], in0=total[:, 0, :], in1=total[:, 1, :], op=ALU.subtract)
+            nc.vector.scalar_tensor_tensor(out=fl[:], in0=fl[:], scalar=10.0, in1=total[:].rearrange("p e q -> p q e"), op0=ALU.mult, op1=ALU.add)
+            nc.vector.scalar_tensor_tensor(out=wanted[:, :, 1], in0=ln[:], scalar=10.0, in1=size[:], op0=ALU.mult, op1=ALU.is_gt)
+            nc.vector.scalar_tensor_tensor(out=fl[:], in0=fl[:], scalar=zrow[:, 1:2], in1=wanted[:], op0=ALU.add, op1=ALU.mult)
+            for h in range(2):
+                nc.vector.tensor_scalar(out=idx[:, :, h, :], in0=fl[:].rearrange("p (j h) e -> p j h e", h=2)[:, :, h, :],
+                                        scalar1=zrow[:, 0:1], scalar2=float(h), op0=ALU.add, op1=ALU.add)
 
         wstage = ctx.enter_context(tc.tile_pool(name="wstage", bufs=1))
         w_sb = wstage.tile([P, NM, C], BF16)
@@ -179,6 +191,9 @@ def tile_coarsepyramid_pa_kernel(tc, feature, segments, w_lr, b_lr, g_lr, be_lr,
             nc.vector.tensor_tensor(out=bsq[:], in0=beta, in1=beta, op=ALU.mult)
             nc.vector.tensor_reduce(out=cc[:, 0:1], in_=beta, axis=AX.X, op=ALU.add)
             nc.vector.tensor_reduce(out=cc[:, 1:2], in_=bsq[:], axis=AX.X, op=ALU.add)
+            cg_ps = opsum.tile([P, 2], F32, name="cg_ps", tag="op")
+            nc.tensor.matmul(out=cg_ps[:], lhsT=ones4[:], rhs=cc[:], start=True, stop=True)
+            live["cg_ps"] = cg_ps
 
         fpool = ctx.enter_context(tc.tile_pool(name="fpool", bufs=2))
         late = ctx.enter_context(tc.tile_pool(name="late", bufs=LATE))
@@ -187,8 +202,7 @@ def tile_coarsepyramid_pa_kernel(tc, feature, segments, w_lr, b_lr, g_lr, be_lr,
         opool = ctx.enter_context(tc.tile_pool(name="opool", bufs=2))
 
         slots = [out_0, out_1]
-        slot_store = [o[0:SLOT_B].rearrange("(h b) (x c) t -> h (b x) (c t)", h=2, c=8).rearrange("h (r k) w -> r h k w", k=TAB)
-                      for o in slots]
+        slot_store = [o[0:SLOT_B].rearrange("b (x c) t -> (b x) (c t)", c=16).rearrange("(r k) w -> r k w", k=TAB) for o in slots]
         slot_rows = [o[0:SLOT_B].rearrange("b (x c) t -> (b x) (c t)", c=8) for o in slots]
 
         def mx_passes(y, pos, hb):
@@ -234,73 +248,94 @@ def tile_coarsepyramid_pa_kernel(tc, feature, segments, w_lr, b_lr, g_lr, be_lr,
                                   in_=x_scales[:, T * b0:T * b0 + n].rearrange("p (b t) -> p b t", b=nb))
             live[("xt", q)] = (xt, xts)
 
-        def piece_sums(q):
+        def piece_sums(q, hb):
             nb = pieces[q][1]
             n = T * nb
             xt, xts = live[("xt", q)]
-            s1 = small.tile([P, NM, 8], F32, name="s1", tag="s1")
-            for hb in range(2):
-                y = ypsum.tile([P, 4, P], F32, name="ysum%d" % hb, tag="y%d" % hb)
-                for i in range(4):
-                    m = 4 * hb + i
-                    for u in range(n // P):
-                        cols = slice(P * u, P * u + P)
-                        nc.tensor.matmul_mx(out=y[:, i, :], lhsT=w_codes[:, m, :].bitcast(FP8X4), lhsT_scale=w_scales[:, m, :],
-                                            rhs=xt[:, cols].bitcast(FP8X4), rhs_scale=xts[:, cols],
-                                            start=u == 0, stop=u == n // P - 1)
-                nc.vector.tensor_reduce(out=s1[:, 4 * hb:4 * hb + 4, 0:nb],
+            if hb == 0:
+                live[("s1", q)] = small.tile([P, NM, 8], F32, name="s1", tag="s1")
+            y = spsum.tile([P, 4, P], F32, name="ysum", tag="ysum")
+            for i in range(4):
+                m = 4 * hb + i
+                for u in range(n // P):
+                    cols = slice(P * u, P * u + P)
+                    nc.tensor.matmul_mx(out=y[:, i, :], lhsT=w_codes[:, m, :].bitcast(FP8X4), lhsT_scale=w_scales[:, m, :],
+                                        rhs=xt[:, cols].bitcast(FP8X4), rhs_scale=xts[:, cols],
+                                        start=u == 0, stop=u == n // P - 1)
+
+            def over_times():
+                nc.vector.tensor_reduce(out=live[("s1", q)][:, 4 * hb:4 * hb + 4, 0:nb],
                                         in_=y[:].rearrange("p m (t b) -> p m b t", b=nb), axis=AX.X, op=ALU.add)
-            live[("s1", q)] = s1
 
-        def chain_a(q):
-            nb = pieces[q][1]
-            s1 = live[("s1", q)]
-            terms = live[("terms", q)]
-            rs = small.tile([P, 16], F32, name="rs", tag="rs")
-            if q == 0:
-                cg_ps = opsum.tile([P, 2], F32, name="cg_ps", tag="op")
-                nc.tensor.matmul(out=cg_ps[:], lhsT=ones4[:], rhs=cc[:], start=True, stop=True)
-                nc.vector.tensor_scalar(out=cg[:], in0=cg_ps[:], scalar1=64.0 / 2048.0, scalar2=None, op0=ALU.mult)
-            nc.vector.scalar_tensor_tensor(out=terms[:, 0:NM, 0:nb], in0=s1[:, :, 0:nb], scalar=2.0,
-                                           in1=beta.unsqueeze(2).to_broadcast([P, NM, nb]), op0=ALU.mult, op1=ALU.mult)
-            nc.vector.tensor_reduce(out=rs[:, 0:nb], in_=s1[:, :, 0:nb].rearrange("p m b -> p b m"), axis=AX.X, op=ALU.add)
-            if q == 0:
-                window_steps()
-            nc.vector.tensor_reduce(out=rs[:, nb:2 * nb], in_=terms[:, :, 0:nb].rearrange("p m b -> p b m"), axis=AX.X, op=ALU.add)
-            st = opsum.tile([P, 16], F32, name="st", tag="op")
-            nc.tensor.matmul(out=st[:, 0:2 * nb], lhsT=ones4[:], rhs=rs[:, 0:2 * nb], start=True, stop=True)
-            live[("st", q)] = st
+            return over_times
 
-        def chain_b(q):
+        def norm_steps(q):
             nb = pieces[q][1]
-            st = live[("st", q)]
-            mv = small.tile([P, 2, 8], F32, name="mv", tag="mv")
-            nc.vector.scalar_tensor_tensor(out=mv[:, :, 0:nb], in0=st[:, 0:2 * nb].rearrange("p (s b) -> p s b", s=2), scalar=1.0 / 2048.0,
-                                           in1=cg[:].unsqueeze(2).to_broadcast([P, 2, nb]), op0=ALU.mult, op1=ALU.add)
-            var = small.tile([P, 8], F32, name="var", tag="var")
-            nc.vector.tensor_tensor(out=var[:, 0:nb], in0=mv[:, 0, 0:nb], in1=mv[:, 0, 0:nb], op=ALU.mult)
-            nc.vector.scalar_tensor_tensor(out=var[:, 0:nb], in0=mv[:, 1, 0:nb], scalar=EPS, in1=var[:, 0:nb], op0=ALU.add, op1=ALU.subtract)
-            std = small.tile([P, 8], F32, name="std", tag="std")
-            nc.scalar.activation(out=std[:, 0:nb], in_=var[:, 0:nb], func=ACT.Sqrt)
-            live[("mv", q)] = mv
-            live[("std", q)] = std
-
-        def chain_c(q):
-            nb = pieces[q][1]
-            mv = live[("mv", q)]
             full = [P, NM, nb]
-            sh = small.tile([P, NM, 8], F32, name="sh", tag="sh")
-            nc.vector.tensor_tensor(out=sh[:, :, 0:nb], in0=beta.unsqueeze(2).to_broadcast(full),
-                                    in1=mv[:, 0, 0:nb].unsqueeze(1).to_broadcast(full), op=ALU.subtract)
+            terms = live[("terms", q)]
+            s1 = live[("s1", q)]
+            rs = small.tile([P, 16], F32, name="rs", tag="rs")
+            st = opsum.tile([P, 16], F32, name="st", tag="op")
+            mv = small.tile([P, 2, 8], F32, name="mv", tag="mv")
+            var = small.tile([P, 8], F32, name="var", tag="var")
+            std = small.tile([P, 8], F32, name="std", tag="std")
             rstd = small.tile([P, 8], F32, name="rstd", tag="rstd")
-            nc.vector.reciprocal(out=rstd[:, 0:nb], in_=live[("std", q)][:, 0:nb])
             sc = small.tile([P, NM, 8], F32, name="sc", tag="sc")
-            nc.vector.tensor_tensor(out=sc[:, :, 0:nb], in0=gamma.unsqueeze(2).to_broadcast(full),
-                                    in1=rstd[:, 0:nb].unsqueeze(1).to_broadcast(full), op=ALU.mult)
-            nc.vector.tensor_tensor(out=sh[:, :, 0:nb], in0=sh[:, :, 0:nb], in1=sc[:, :, 0:nb], op=ALU.mult)
-            nc.vector.tensor_tensor(out=sh[:, :, 0:nb], in0=sh[:, :, 0:nb], in1=shift0.unsqueeze(2).to_broadcast(full), op=ALU.add)
+            sh = small.tile([P, NM, 8], F32, name="sh", tag="sh")
             live[("sc", q)] = sc
             live[("sh", q)] = sh
+
+            def bias_terms():
+                nc.vector.scalar_tensor_tensor(out=terms[:, 0:NM, 0:nb], in0=s1[:, :, 0:nb], scalar=2.0,
+                                               in1=beta.unsqueeze(2).to_broadcast(full), op0=ALU.mult, op1=ALU.mult)
+
+            def over_tiles(part, src):
+                nc.vector.tensor_reduce(out=rs[:, part * nb:part * nb + nb], in_=src.rearrange("p m b -> p b m"), axis=AX.X, op=ALU.add)
+
+            def squares_over_tiles():
+                over_tiles(1, terms[:, :, 0:nb])
+                nc.tensor.matmul(out=st[:, 0:2 * nb], lhsT=ones4[:], rhs=rs[:, 0:2 * nb], start=True, stop=True)
+
+            def moments():
+                nc.vector.scalar_tensor_tensor(out=mv[:, :, 0:nb], in0=st[:, 0:2 * nb].rearrange("p (s b) -> p s b", s=2),
+                                               scalar=1.0 / 2048.0, in1=cg[:].unsqueeze(2).to_broadcast([P, 2, nb]),
+                                               op0=ALU.mult, op1=ALU.add)
+
+            def mean_squared():
+                nc.vector.tensor_tensor(out=var[:, 0:nb], in0=mv[:, 0, 0:nb], in1=mv[:, 0, 0:nb], op=ALU.mult)
+
+            def deviation():
+                nc.vector.scalar_tensor_tensor(out=var[:, 0:nb], in0=mv[:, 1, 0:nb], scalar=EPS, in1=var[:, 0:nb],
+                                               op0=ALU.add, op1=ALU.subtract)
+                nc.scalar.activation(out=std[:, 0:nb], in_=var[:, 0:nb], func=ACT.Sqrt)
+
+            def shift_a():
+                nc.vector.tensor_tensor(out=sh[:, :, 0:nb], in0=beta.unsqueeze(2).to_broadcast(full),
+                                        in1=mv[:, 0, 0:nb].unsqueeze(1).to_broadcast(full), op=ALU.subtract)
+
+            def inverse():
+                nc.vector.reciprocal(out=rstd[:, 0:nb], in_=std[:, 0:nb])
+
+            def scale():
+                nc.vector.tensor_tensor(out=sc[:, :, 0:nb], in0=gamma.unsqueeze(2).to_broadcast(full),
+                                        in1=rstd[:, 0:nb].unsqueeze(1).to_broadcast(full), op=ALU.mult)
+
+            def shift_b():
+                nc.vector.tensor_tensor(out=sh[:, :, 0:nb], in0=sh[:, :, 0:nb], in1=sc[:, :, 0:nb], op=ALU.mult)
+
+            def shift_c():
+                nc.vector.tensor_tensor(out=sh[:, :, 0:nb], in0=sh[:, :, 0:nb], in1=shift0.unsqueeze(2).to_broadcast(full), op=ALU.add)
+
+            return [bias_terms, lambda: over_tiles(0, s1[:, :, 0:nb]), squares_over_tiles,
+                    moments, mean_squared, deviation, shift_a, inverse, scale, shift_b, shift_c]
+
+        def next_step():
+            if live["steps"]:
+                live["steps"].pop(0)()
+
+        def all_steps():
+            while live["steps"]:
+                next_step()
 
         def main_mx(pos):
             ys = []
@@ -342,7 +377,7 @@ def tile_coarsepyramid_pa_kernel(tc, feature, segments, w_lr, b_lr, g_lr, be_lr,
                     live[("f2", pos)] = late.tile([P, 2, NM, T], F32, name="f2_late", tag="f2_late")
                 else:
                     live[("f2", pos)] = opool.tile([P, 2, NM, T], F32, name="f2", tag="f2")
-            nc.scalar.copy(out=live[("f2", pos)][:, l, :, :].rearrange("p (j mm) t -> p j mm t", mm=2),
+            nc.vector.tensor_copy(out=live[("f2", pos)][:, l, :, :].rearrange("p (j mm) t -> p j mm t", mm=2),
                            in_=live[("f", pos)][:, :, :, T * l:T * l + T].rearrange("p mm j t -> p j mm t"))
 
         def store_feat(pos):
@@ -363,6 +398,7 @@ def tile_coarsepyramid_pa_kernel(tc, feature, segments, w_lr, b_lr, g_lr, be_lr,
 
         def window(out, in_, shift, n):
             nc.vector.tensor_tensor(out=out, in0=in_[:, :, :, 0:n], in1=in_[:, :, :, shift:shift + n], op=ALU.max)
+            next_step()
 
         def pairs_up(pos):
             for mm in range(2):
@@ -380,39 +416,38 @@ def tile_coarsepyramid_pa_kernel(tc, feature, segments, w_lr, b_lr, g_lr, be_lr,
             u, first = k // 2, k % 2 == 0
             if first:
                 n = 2 if k < TAB - 1 else 1
-                live[("r", pos, u)] = rpool.tile([P, 2, n, 2, 4, 64], F32, name="r%d" % u, tag="r%d" % u)
+                live[("r", pos, u)] = rpool.tile([P, n, 2, 2, 4, 64], F32, name="r%d" % u, tag="r%d" % u)
             r = live[("r", pos, u)]
             for mm in range(2):
                 tp = tpsum.tile([P, 4, P], F32, name="tp", tag="tp")
                 for j in range(4):
                     src = live[("f", pos)][:, mm, j, :] if k == 0 else tab[:, k - 1, mm, j, :]
                     nc.tensor.transpose(tp[:, j, :], src, ident[:])
-                dst = r[:, :, k % 2, mm, :, :]
+                dst = r[:, k % 2, :, mm, :, :]
                 rows = tp[:].rearrange("p j (h q) -> p h j q", h=2)
                 if k == TAB - 1:
                     nc.vector.tensor_copy(out=dst, in_=rows)
                 else:
                     nc.scalar.copy(out=dst, in_=rows)
 
-        def store_rows(pos, u, h):
+        def store_rows(pos, u):
             r = live[("r", pos, u)]
-            nc.sync.dma_start(out=slot_store[pos % 2][:, h, 2 * u:min(2 * u + 2, TAB), :],
-                              in_=r[:, h, :, :, :, :].rearrange("p k mm j q -> p k (mm j q)"))
+            nc.sync.dma_start(out=slot_store[pos % 2][:, 2 * u:min(2 * u + 2, TAB), :],
+                              in_=r[:].rearrange("p k h mm j q -> p k (h mm j q)"))
 
         def gathers(pos):
             j = order[pos]
             got = {}
-            for h in (1, 0):
-                rows = slot_rows[pos % 2][0:128 * TAB * (h + 1), :]
+            for h in range(2):
                 for e in range(2):
                     g = gpool.tile([P, C], F32, name="g%d%d" % (h, e), tag="g%d%d" % (h, e), bufs=3)
-                    nc.gpsimd.indirect_dma_start(out=g[:], out_offset=None, in_=rows,
+                    nc.gpsimd.indirect_dma_start(out=g[:], out_offset=None, in_=slot_rows[pos % 2],
                                                  in_offset=bass.IndirectOffsetOnAxis(ap=idx[:, j, h, e:e + 1], axis=0))
                     got[(h, e)] = g
             live[("g", pos)] = got
 
         def window_max(pos, h):
-            if h == 1:
+            if h == 0:
                 live[("gc", pos)] = gpool.tile([P, NM, 2, 64], F32, name="gc", tag="gc")
             got = live[("g", pos)]
             nc.vector.tensor_tensor(out=live[("gc", pos)][:, :, h, :], in0=got[(h, 0)][:].rearrange("p (m q) -> p m q", m=NM),
@@ -432,12 +467,15 @@ def tile_coarsepyramid_pa_kernel(tc, feature, segments, w_lr, b_lr, g_lr, be_lr,
             for i in range(4):
                 nc.tensor.transpose(op[:, i, :], gc[:, 4 * (i % 2) + 2 * hb + i // 2, :, :].rearrange("p h q -> p (h q)"), ident[:])
             nc.scalar.copy(out=o[:, :, 4 * hb:4 * hb + 4, :], in_=op[:].rearrange("p m (l n) -> p l m n", l=2))
-            if hb == 1:
-                dst = out_1[2 * j:2 * j + 2].rearrange("l (p m) n -> p l (m n)", m=NM)
-                if is_late:
-                    send(1, dst, o[:].rearrange("p l m n -> p l (m n)"))
-                else:
-                    nc.sync.dma_start(out=dst, in_=o[:].rearrange("p l m n -> p l (m n)"))
+
+        def store_pooled(pos):
+            j = order[pos]
+            dst = out_1[2 * j:2 * j + 2].rearrange("l (p m) n -> p l (m n)", m=NM)
+            src = live[("o", pos)][:].rearrange("p l m n -> p l (m n)")
+            if j < LATE:
+                send(1, dst, src)
+            else:
+                nc.sync.dma_start(out=dst, in_=src)
 
         def group_all(q):
             for b in range(0, pieces[q][1], 2):
@@ -449,73 +487,82 @@ def tile_coarsepyramid_pa_kernel(tc, feature, segments, w_lr, b_lr, g_lr, be_lr,
             first = a < NCH
             second = 0 <= c < NCH
             third = 0 <= w < NCH
-            starts = [q for q in range(1, len(pieces)) if first_use(q) == a]
+            early = {1: (1, 1, 1, 1, 1, 2), 2: (2, 2, 2, 3, 3, 3), 3: (3, 3, 3, 4, 4, 5)}
+
+            def at(q, stage):
+                return early[q][stage] if q in early else first_use(q) - (0, 5, 4, 3, 2, 1)[stage]
+
+            def due(stage):
+                return [q for q in range(1, len(pieces)) if at(q, stage) == a]
+
             if second:
                 rows_out(c, 0)
                 pairs_up(c)
-            if a >= 4:
-                squares(a + 3)
+            if a > 1:
+                squares(min(2 * a - 1, a + 4))
             for q in range(1, len(pieces)):
-                if a == (first_use(q) - 4 if q > 3 else q):
+                if q in early and a == at(q, 0):
                     group_all(q)
+                if q not in early:
+                    b = 2 * (a - at(q, 1)) + pieces[q][1] - 2
+                    if 0 <= b < pieces[q][1]:
+                        group_piece(q, b)
+            if a != at(2, 5):
+                for q in due(5):
+                    live["steps"] += norm_steps(q)
             if second:
                 level_up(c, 0)
                 rows_out(c, 1)
-                store_rows(c, 0, 1)
-                store_rows(c, 0, 0)
-                copy_feat(c, 0)
-                copy_feat(c, 1)
-                store_feat(c)
-            for q in starts:
-                piece_sums(q)
-                chain_a(q)
+                store_rows(c, 0)
             if third:
-                window_max(w, 1)
+                window_max(w, 0)
             if second:
                 level_up(c, 1)
                 rows_out(c, 2)
-            for q in range(1, len(pieces)):
-                if a == (first_use(q) - 4 if q > 3 else q):
-                    quantise_piece(q)
-                if a == first_use(q) - 1:
-                    reorder_codes(q)
-            for q in starts:
-                chain_b(q)
+            for q in due(1):
+                quantise_piece(q)
+            for q in due(2):
+                reorder_codes(q)
             if third:
-                window_max(w, 0)
+                window_max(w, 1)
                 if w >= NCH - 2:
                     give_up_slot(w % 2)
-            if second:
-                level_up(c, 2)
-            for q in starts:
-                chain_c(q)
-            if second:
-                rows_out(c, 3)
-                store_rows(c, 1, 1)
-                store_rows(c, 1, 0)
             if first:
                 main_mx(a)
+            if second:
+                level_up(c, 2)
+                rows_out(c, 3)
+                store_rows(c, 1)
+            if any(first_use(q) == a for q in range(1, len(pieces))):
+                all_steps()
+            if first:
                 apply_norm(a, 0)
                 apply_norm(a, 1)
+            for hb in range(2):
+                for q in due(3 + hb):
+                    live["steps"].append(piece_sums(q, hb))
+            if a == at(2, 5):
+                live["steps"] += norm_steps(2)
+            if third:
+                pooled_out(w, 0)
+                pooled_out(w, 1)
             if second:
                 level_up(c, 3)
                 level_up(c, 4)
                 rows_out(c, 4)
-                store_rows(c, 2, 1)
-                store_rows(c, 2, 0)
+                store_rows(c, 2)
                 gathers(c)
-            if third:
-                pooled_out(w, 0)
-                pooled_out(w, 1)
-            for q in range(1, len(pieces)):
-                p0 = first_use(q)
-                if a == (p0 - 7 if q > 3 else max(q - 2, 0)) and q > 1:
-                    load_piece(q)
-            if a in (1, 2):
+            if 1 <= a <= 4:
                 squares(2 * a)
-                squares(2 * a + 1)
-            if a == 3:
-                squares(6)
+            if third:
+                store_pooled(w)
+            if second:
+                copy_feat(c, 0)
+                copy_feat(c, 1)
+                store_feat(c)
+            for q in range(2, len(pieces)):
+                if a == (max(first_use(q) - 10, 1) if q not in early else q - 2):
+                    load_piece(q)
 
         step_constants()
         warm = const.tile([P, 1], F32)
@@ -527,12 +574,16 @@ def tile_coarsepyramid_pa_kernel(tc, feature, segments, w_lr, b_lr, g_lr, be_lr,
         reorder_codes(0)
         quantise_w(0)
         quantise_w(1)
-        piece_sums(0)
+        piece_sums(0, 0)()
+        piece_sums(0, 1)()
         squares(0)
         squares(1)
-        chain_a(0)
-        chain_b(0)
-        chain_c(0)
+        live["steps"] = norm_steps(0)
+        next_step()
+        next_step()
+        nc.vector.tensor_scalar(out=cg[:], in0=live["cg_ps"][:], scalar1=64.0 / 2048.0, scalar2=None, op0=ALU.mult)
+        window_steps()
+        all_steps()
         window_rows()
         for a in range(NCH + 4):
             one_round(a)

@@ -27,6 +27,7 @@ ZERO = TOP + 2 * N_OK[5]
 EPS = 1e-5
 SLOT_B = 10
 LATE = SLOT_B // 2
+FOUR = 12
 FLOPS = 2 * B * C2 * C * T
 
 
@@ -37,15 +38,14 @@ def tile_coarsepyramid_pa_kernel(tc, feature, segments, w_lr, b_lr, g_lr, be_lr,
         small = ctx.enter_context(tc.tile_pool(name="small", bufs=3))
         stage = ctx.enter_context(tc.tile_pool(name="stage", bufs=2))
         ypsum = ctx.enter_context(tc.psum_pool(name="ypsum", bufs=1))
-        tpsum = ctx.enter_context(tc.psum_pool(name="tpsum", bufs=3))
+        tpsum = ctx.enter_context(tc.psum_pool(name="tpsum", bufs=4))
         opsum = ctx.enter_context(tc.psum_pool(name="opsum", bufs=2))
-        spsum = ctx.enter_context(tc.psum_pool(name="spsum", bufs=1))
 
-        order = list(range(LATE, NCH)) + list(range(LATE))
+        order = list(range(2 * LATE, NCH)) + list(range(LATE, 2 * LATE)) + list(range(LATE))
         live = {"steps": []}
         held = {0: [], 1: []}
 
-        pieces = [(10, 4), (14, 4), (18, 4), (22, 8), (30, 8), (38, 8), (46, 2), (0, 8), (8, 2)]
+        pieces = [(20, 4), (24, 4), (28, 4), (32, 8), (40, 8), (10, 8), (18, 2), (0, 8), (8, 2)]
         x_codes = const.tile([P, B * T], U32, align_bytes=64)
         x_scales = const.tile([P, B * T], U8, align_bytes=64)
 
@@ -96,6 +96,7 @@ def tile_coarsepyramid_pa_kernel(tc, feature, segments, w_lr, b_lr, g_lr, be_lr,
         nc.gpsimd.iota(pid[:], pattern=[[0, 1]], base=0, channel_multiplier=1)
         make_identity(nc, ident[:])
         make_block_diagonal(nc, ones4[:], 4)
+        ctx.enter_context(tc.manual_schedule())
 
         def step_constants():
             for k in range(NS):
@@ -146,6 +147,8 @@ def tile_coarsepyramid_pa_kernel(tc, feature, segments, w_lr, b_lr, g_lr, be_lr,
             nc.vector.scalar_tensor_tensor(out=fl[:], in0=fl[:], scalar=10.0, in1=total[:].rearrange("p e q -> p q e"), op0=ALU.mult, op1=ALU.add)
             nc.vector.scalar_tensor_tensor(out=wanted[:, :, 1], in0=ln[:], scalar=10.0, in1=size[:], op0=ALU.mult, op1=ALU.is_gt)
             nc.vector.scalar_tensor_tensor(out=fl[:], in0=fl[:], scalar=zrow[:, 1:2], in1=wanted[:], op0=ALU.add, op1=ALU.mult)
+            second = fl[:].rearrange("p (j h) e -> p j h e", h=2)[:, SLOT_B + 1:SLOT_B + FOUR:2, :, :]
+            nc.vector.tensor_scalar(out=second, in0=second, scalar1=float(2 * TAB * P), scalar2=None, op0=ALU.add)
             for h in range(2):
                 nc.vector.tensor_scalar(out=idx[:, :, h, :], in0=fl[:].rearrange("p (j h) e -> p j h e", h=2)[:, :, h, :],
                                         scalar1=zrow[:, 0:1], scalar2=float(h), op0=ALU.add, op1=ALU.add)
@@ -201,9 +204,17 @@ def tile_coarsepyramid_pa_kernel(tc, feature, segments, w_lr, b_lr, g_lr, be_lr,
         gpool = ctx.enter_context(tc.tile_pool(name="gpool", bufs=2))
         opool = ctx.enter_context(tc.tile_pool(name="opool", bufs=2))
 
-        slots = [out_0, out_1]
-        slot_store = [o[0:SLOT_B].rearrange("b (x c) t -> (b x) (c t)", c=16).rearrange("(r k) w -> r k w", k=TAB) for o in slots]
-        slot_rows = [o[0:SLOT_B].rearrange("b (x c) t -> (b x) (c t)", c=8) for o in slots]
+        def slot_of(pos):
+            x, second = (pos // 2 % 2, pos % 2) if pos < FOUR else (pos % 2, 0)
+            return (out_0, out_1)[x], second
+
+        def slot_store(pos):
+            o, second = slot_of(pos)
+            return o[SLOT_B * second:SLOT_B * (second + 1)].rearrange("b (x c) t -> (b x) (c t)", c=16).rearrange("(r k) w -> r k w", k=TAB)
+
+        def slot_rows(pos):
+            o, second = slot_of(pos)
+            return o[0:SLOT_B * (second + 1)].rearrange("b (x c) t -> (b x) (c t)", c=8)
 
         def mx_passes(y, pos, hb):
             cols = slice(P * order[pos], P * order[pos] + P)
@@ -225,6 +236,7 @@ def tile_coarsepyramid_pa_kernel(tc, feature, segments, w_lr, b_lr, g_lr, be_lr,
             q, bi = group_of(pos)
             if bi == 0:
                 live[("terms", q)] = small.tile([P, NM + 2, 8], F32, name="terms", tag="terms")
+                live[("s1", q)] = small.tile([P, NM, 8], F32, name="s1", tag="s1")
             terms = live[("terms", q)]
             ys = []
             for hb in range(2):
@@ -232,42 +244,13 @@ def tile_coarsepyramid_pa_kernel(tc, feature, segments, w_lr, b_lr, g_lr, be_lr,
                 mx_passes(y, pos, hb)
                 ys.append(y)
             for hb in range(2):
+                nc.vector.tensor_reduce(out=live[("s1", q)][:, 4 * hb:4 * hb + 4, bi:bi + 2],
+                                        in_=ys[hb][:].rearrange("p m (l t) -> p m l t", l=2), axis=AX.X, op=ALU.add)
+            for hb in range(2):
                 junk = small.tile([P, 4, T], F32, name="junk", tag="junk")
                 for l in range(2):
                     nc.scalar.activation(out=junk[:], in_=ys[hb][:, :, T * l:T * l + T], func=ACT.Square,
                                          accum_out=terms[:, NM + hb, bi + l:bi + l + 1])
-
-        def reorder_codes(q):
-            b0, nb = pieces[q]
-            n = T * nb
-            xt = stage.tile([P, 8 * T], U32, align_bytes=64, name="xt", tag="xt")
-            xts = stage.tile([P, 8 * T], U8, align_bytes=64, name="xts", tag="xts")
-            nc.vector.tensor_copy(out=xt[:, 0:n].bitcast(I32).rearrange("p (t b) -> p t b", b=nb),
-                                  in_=x_codes[:, T * b0:T * b0 + n].bitcast(I32).rearrange("p (b t) -> p t b", b=nb))
-            nc.vector.tensor_copy(out=xts[:, 0:n].rearrange("p (t b) -> p b t", b=nb),
-                                  in_=x_scales[:, T * b0:T * b0 + n].rearrange("p (b t) -> p b t", b=nb))
-            live[("xt", q)] = (xt, xts)
-
-        def piece_sums(q, hb):
-            nb = pieces[q][1]
-            n = T * nb
-            xt, xts = live[("xt", q)]
-            if hb == 0:
-                live[("s1", q)] = small.tile([P, NM, 8], F32, name="s1", tag="s1")
-            y = spsum.tile([P, 4, P], F32, name="ysum", tag="ysum")
-            for i in range(4):
-                m = 4 * hb + i
-                for u in range(n // P):
-                    cols = slice(P * u, P * u + P)
-                    nc.tensor.matmul_mx(out=y[:, i, :], lhsT=w_codes[:, m, :].bitcast(FP8X4), lhsT_scale=w_scales[:, m, :],
-                                        rhs=xt[:, cols].bitcast(FP8X4), rhs_scale=xts[:, cols],
-                                        start=u == 0, stop=u == n // P - 1)
-
-            def over_times():
-                nc.vector.tensor_reduce(out=live[("s1", q)][:, 4 * hb:4 * hb + 4, 0:nb],
-                                        in_=y[:].rearrange("p m (t b) -> p m b t", b=nb), axis=AX.X, op=ALU.add)
-
-            return over_times
 
         def norm_steps(q):
             nb = pieces[q][1]
@@ -432,7 +415,7 @@ def tile_coarsepyramid_pa_kernel(tc, feature, segments, w_lr, b_lr, g_lr, be_lr,
 
         def store_rows(pos, u):
             r = live[("r", pos, u)]
-            nc.sync.dma_start(out=slot_store[pos % 2][:, 2 * u:min(2 * u + 2, TAB), :],
+            nc.sync.dma_start(out=slot_store(pos)[:, 2 * u:min(2 * u + 2, TAB), :],
                               in_=r[:].rearrange("p k h mm j q -> p k (h mm j q)"))
 
         def gathers(pos):
@@ -441,7 +424,7 @@ def tile_coarsepyramid_pa_kernel(tc, feature, segments, w_lr, b_lr, g_lr, be_lr,
             for h in range(2):
                 for e in range(2):
                     g = gpool.tile([P, C], F32, name="g%d%d" % (h, e), tag="g%d%d" % (h, e), bufs=3)
-                    nc.gpsimd.indirect_dma_start(out=g[:], out_offset=None, in_=slot_rows[pos % 2],
+                    nc.gpsimd.indirect_dma_start(out=g[:], out_offset=None, in_=slot_rows(pos),
                                                  in_offset=bass.IndirectOffsetOnAxis(ap=idx[:, j, h, e:e + 1], axis=0))
                     got[(h, e)] = g
             live[("g", pos)] = got
@@ -487,10 +470,10 @@ def tile_coarsepyramid_pa_kernel(tc, feature, segments, w_lr, b_lr, g_lr, be_lr,
             first = a < NCH
             second = 0 <= c < NCH
             third = 0 <= w < NCH
-            early = {1: (1, 1, 1, 1, 1, 2), 2: (2, 2, 2, 3, 3, 3), 3: (3, 3, 3, 4, 4, 5)}
+            early = {1: (1, 2), 2: (2, 3), 3: (3, 5)}
 
             def at(q, stage):
-                return early[q][stage] if q in early else first_use(q) - (0, 5, 4, 3, 2, 1)[stage]
+                return early[q][stage] if q in early else first_use(q) - (5, 1)[stage]
 
             def due(stage):
                 return [q for q in range(1, len(pieces)) if at(q, stage) == a]
@@ -504,12 +487,11 @@ def tile_coarsepyramid_pa_kernel(tc, feature, segments, w_lr, b_lr, g_lr, be_lr,
                 if q in early and a == at(q, 0):
                     group_all(q)
                 if q not in early:
-                    b = 2 * (a - at(q, 1)) + pieces[q][1] - 2
+                    b = 2 * (a - at(q, 0)) + pieces[q][1] - 2
                     if 0 <= b < pieces[q][1]:
                         group_piece(q, b)
-            if a != at(2, 5):
-                for q in due(5):
-                    live["steps"] += norm_steps(q)
+            for q in due(1):
+                live["steps"] += norm_steps(q)
             if second:
                 level_up(c, 0)
                 rows_out(c, 1)
@@ -519,10 +501,8 @@ def tile_coarsepyramid_pa_kernel(tc, feature, segments, w_lr, b_lr, g_lr, be_lr,
             if second:
                 level_up(c, 1)
                 rows_out(c, 2)
-            for q in due(1):
+            for q in due(0):
                 quantise_piece(q)
-            for q in due(2):
-                reorder_codes(q)
             if third:
                 window_max(w, 1)
                 if w >= NCH - 2:
@@ -538,17 +518,14 @@ def tile_coarsepyramid_pa_kernel(tc, feature, segments, w_lr, b_lr, g_lr, be_lr,
             if first:
                 apply_norm(a, 0)
                 apply_norm(a, 1)
-            for hb in range(2):
-                for q in due(3 + hb):
-                    live["steps"].append(piece_sums(q, hb))
-            if a == at(2, 5):
-                live["steps"] += norm_steps(2)
             if third:
                 pooled_out(w, 0)
                 pooled_out(w, 1)
             if second:
                 level_up(c, 3)
                 level_up(c, 4)
+                copy_feat(c, 0)
+                copy_feat(c, 1)
                 rows_out(c, 4)
                 store_rows(c, 2)
                 gathers(c)
@@ -557,8 +534,6 @@ def tile_coarsepyramid_pa_kernel(tc, feature, segments, w_lr, b_lr, g_lr, be_lr,
             if third:
                 store_pooled(w)
             if second:
-                copy_feat(c, 0)
-                copy_feat(c, 1)
                 store_feat(c)
             for q in range(2, len(pieces)):
                 if a == (max(first_use(q) - 10, 1) if q not in early else q - 2):
@@ -571,11 +546,8 @@ def tile_coarsepyramid_pa_kernel(tc, feature, segments, w_lr, b_lr, g_lr, be_lr,
         group_all(0)
         quantise_piece(0)
         norm_constants()
-        reorder_codes(0)
         quantise_w(0)
         quantise_w(1)
-        piece_sums(0, 0)()
-        piece_sums(0, 1)()
         squares(0)
         squares(1)
         live["steps"] = norm_steps(0)

@@ -360,8 +360,12 @@ def tile_coarsepyramid_pa_kernel(tc, feature, segments, w_lr, b_lr, g_lr, be_lr,
                     live[("f2", pos)] = late.tile([P, 2, NM, T], F32, name="f2_late", tag="f2_late")
                 else:
                     live[("f2", pos)] = opool.tile([P, 2, NM, T], F32, name="f2", tag="f2")
-            nc.vector.tensor_copy(out=live[("f2", pos)][:, l, :, :].rearrange("p (j mm) t -> p j mm t", mm=2),
-                           in_=live[("f", pos)][:, :, :, T * l:T * l + T].rearrange("p mm j t -> p j mm t"))
+            out = live[("f2", pos)][:, l, :, :].rearrange("p (j mm) t -> p j mm t", mm=2)
+            src = live[("f", pos)][:, :, :, T * l:T * l + T].rearrange("p mm j t -> p j mm t")
+            if l == 0:
+                nc.scalar.copy(out=out, in_=src)
+            else:
+                nc.vector.tensor_tensor(out=out, in0=src, in1=src, op=ALU.max)
 
         def store_feat(pos):
             j = order[pos]
@@ -420,21 +424,18 @@ def tile_coarsepyramid_pa_kernel(tc, feature, segments, w_lr, b_lr, g_lr, be_lr,
 
         def gathers(pos):
             j = order[pos]
-            got = {}
+            got = [gpool.tile([P, 2, C], F32, name="g%d" % e, tag="g%d" % e, bufs=3) for e in range(2)]
             for h in range(2):
                 for e in range(2):
-                    g = gpool.tile([P, C], F32, name="g%d%d" % (h, e), tag="g%d%d" % (h, e), bufs=3)
-                    nc.gpsimd.indirect_dma_start(out=g[:], out_offset=None, in_=slot_rows(pos),
+                    nc.gpsimd.indirect_dma_start(out=got[e][:, h, :], out_offset=None, in_=slot_rows(pos),
                                                  in_offset=bass.IndirectOffsetOnAxis(ap=idx[:, j, h, e:e + 1], axis=0))
-                    got[(h, e)] = g
             live[("g", pos)] = got
 
-        def window_max(pos, h):
-            if h == 0:
-                live[("gc", pos)] = gpool.tile([P, NM, 2, 64], F32, name="gc", tag="gc")
-            got = live[("g", pos)]
-            nc.vector.tensor_tensor(out=live[("gc", pos)][:, :, h, :], in0=got[(h, 0)][:].rearrange("p (m q) -> p m q", m=NM),
-                                    in1=got[(h, 1)][:].rearrange("p (m q) -> p m q", m=NM), op=ALU.max)
+        def window_max(pos):
+            gc = gpool.tile([P, NM, 2, 64], F32, name="gc", tag="gc")
+            got = [x[:].rearrange("p h (m q) -> p h m q", m=NM) for x in live[("g", pos)]]
+            nc.vector.tensor_tensor(out=gc[:].rearrange("p m h q -> p h m q"), in0=got[0], in1=got[1], op=ALU.max)
+            live[("gc", pos)] = gc
 
         def pooled_out(pos, hb):
             j = order[pos]
@@ -496,15 +497,13 @@ def tile_coarsepyramid_pa_kernel(tc, feature, segments, w_lr, b_lr, g_lr, be_lr,
                 level_up(c, 0)
                 rows_out(c, 1)
                 store_rows(c, 0)
-            if third:
-                window_max(w, 0)
             if second:
                 level_up(c, 1)
                 rows_out(c, 2)
             for q in due(0):
                 quantise_piece(q)
             if third:
-                window_max(w, 1)
+                window_max(w)
                 if w >= NCH - 2:
                     give_up_slot(w % 2)
             if first:

@@ -362,10 +362,7 @@ def tile_coarsepyramid_pa_kernel(tc, feature, segments, w_lr, b_lr, g_lr, be_lr,
                     live[("f2", pos)] = opool.tile([P, 2, NM, T], F32, name="f2", tag="f2")
             out = live[("f2", pos)][:, l, :, :].rearrange("p (j mm) t -> p j mm t", mm=2)
             src = live[("f", pos)][:, :, :, T * l:T * l + T].rearrange("p mm j t -> p j mm t")
-            if l == 0:
-                nc.scalar.copy(out=out, in_=src)
-            else:
-                nc.vector.tensor_tensor(out=out, in0=src, in1=src, op=ALU.max)
+            nc.scalar.copy(out=out, in_=src)
 
         def store_feat(pos):
             j = order[pos]
@@ -412,10 +409,16 @@ def tile_coarsepyramid_pa_kernel(tc, feature, segments, w_lr, b_lr, g_lr, be_lr,
                     nc.tensor.transpose(tp[:, j, :], src, ident[:])
                 dst = r[:, k % 2, :, mm, :, :]
                 rows = tp[:].rearrange("p j (h q) -> p h j q", h=2)
-                if k == TAB - 1:
+                if k == TAB - 2 and mm == 1:
+                    live["late_copy"] = (dst, rows)
+                elif k == TAB - 1:
                     nc.vector.tensor_copy(out=dst, in_=rows)
                 else:
                     nc.scalar.copy(out=dst, in_=rows)
+
+        def late_copy():
+            dst, rows = live["late_copy"]
+            nc.vector.tensor_copy(out=dst, in_=rows)
 
         def store_rows(pos, u):
             r = live[("r", pos, u)]
@@ -511,7 +514,6 @@ def tile_coarsepyramid_pa_kernel(tc, feature, segments, w_lr, b_lr, g_lr, be_lr,
             if second:
                 level_up(c, 2)
                 rows_out(c, 3)
-                store_rows(c, 1)
             if any(first_use(q) == a for q in range(1, len(pieces))):
                 all_steps()
             if first:
@@ -523,6 +525,8 @@ def tile_coarsepyramid_pa_kernel(tc, feature, segments, w_lr, b_lr, g_lr, be_lr,
             if second:
                 level_up(c, 3)
                 level_up(c, 4)
+                late_copy()
+                store_rows(c, 1)
                 copy_feat(c, 0)
                 copy_feat(c, 1)
                 rows_out(c, 4)

from contextlib import ExitStack

import concourse.bass as bass
import concourse.mybir as mybir
from concourse.masks import make_block_diagonal, make_identity

F32 = mybir.dt.float32
BF16 = mybir.dt.bfloat16
I32 = mybir.dt.int32
U32 = mybir.dt.uint32
U8 = mybir.dt.uint8
FP8X4 = mybir.dt.float8_e4m3fn_x4
ALU = mybir.AluOpType
ACT = mybir.ActivationFunctionType
AX = mybir.AxisListType

P = 128
B, C, T, C2 = 48, 512, 64, 1024
NM = 8
NCH = B // 2
SIZES = [1, 3, 6, 12, 24, 48]
LEV = len(SIZES)
N_OK = [T - w + 1 for w in SIZES]
TAB = 5
TOP = 2 * N_OK[4]
ZERO = TOP + 2 * N_OK[5]
EPS = 1e-5
SLOT_B = 10
LATE = SLOT_B // 2
FOUR = 12
FLOPS = 2 * B * C2 * C * T


def tile_coarsepyramid_pa_kernel(tc, feature, segments, w_lr, b_lr, g_lr, be_lr, out_0, out_1):
    nc = tc.nc
    with ExitStack() as ctx:
        const = ctx.enter_context(tc.tile_pool(name="const", bufs=1))
        small = ctx.enter_context(tc.tile_pool(name="small", bufs=3))
        stage = ctx.enter_context(tc.tile_pool(name="stage", bufs=2))
        ypsum = ctx.enter_context(tc.psum_pool(name="ypsum", bufs=1))
        tpsum = ctx.enter_context(tc.psum_pool(name="tpsum", bufs=4))
        opsum = ctx.enter_context(tc.psum_pool(name="opsum", bufs=2))

        order = list(range(2 * LATE, NCH)) + list(range(LATE, 2 * LATE)) + list(range(LATE))
        live = {"steps": []}
        held = {0: [], 1: []}

        pieces = [(20, 4), (24, 4), (28, 4), (32, 8), (40, 8), (10, 8), (18, 2), (0, 8), (8, 2)]
        x_codes = const.tile([P, B * T], U32, align_bytes=64)
        x_scales = const.tile([P, B * T], U8, align_bytes=64)

        def first_use(q):
            return order.index(pieces[q][0] // 2)

        def load_piece(q):
            b0, nb = pieces[q]
            raw = stage.tile([P, 8, 4, T], BF16, name="raw", tag="raw", bufs=3)
            nc.sync.dma_start(out=raw[:, 0:nb, :, :].rearrange("p b j t -> p b (j t)"),
                              in_=feature[b0:b0 + nb].rearrange("b (p j) t -> p b (j t)", j=4))
            live[("raw", q)] = raw

        def group_piece(q, b):
            raw = live[("raw", q)]
            if b == 0:
                live[("x_grp", q)] = stage.tile([P, 8, T, 4], BF16, align_bytes=64, name="x_grp", tag="x_grp")
            x_grp = live[("x_grp", q)]
            if q == 0:
                nc.vector.tensor_copy(out=x_grp[:, b:b + 2, :, :], in_=raw[:, b:b + 2, :, :].rearrange("p b j t -> p b t j"))
            else:
                nc.scalar.copy(out=x_grp[:, b:b + 2, :, :], in_=raw[:, b:b + 2, :, :].rearrange("p b j t -> p b t j"))

        def quantise_piece(q):
            b0, nb = pieces[q]
            x_grp = live[("x_grp", q)]
            nc.vector.quantize_mx(out=x_codes[:, T * b0:T * (b0 + nb)].bitcast(FP8X4),
                                  scales=x_scales[:, T * b0:T * (b0 + nb)],
                                  in_=x_grp[:, 0:nb, :, :].rearrange("p b t j -> p (b t j)"))

        w_codes = const.tile([P, NM, P], U32, align_bytes=64)
        w_scales = const.tile([P, NM, P], U8, align_bytes=64)
        vec_bf = [const.tile([P, NM], BF16, name="vec_bf%d" % i) for i in range(3)]
        beta, gamma, shift0 = [v[:] for v in vec_bf]
        seg_bf = const.tile([P, NCH, 2, 2], BF16)
        ident = const.tile([P, P], F32)
        ones4 = const.tile([P, P], F32)
        tab = const.tile([P, TAB - 1, 2, 4, P], F32)
        pairs = const.tile([P, 2, 4, 2 * (T - 1)], F32)
        STEPS = [-1000.0] + [float(w - 1) for w in SIZES[1:]]
        NS = len(STEPS)
        thr = const.tile([P, NS], F32)
        gain = const.tile([P, 2, NS], F32)
        pid = const.tile([P, 1], I32)
        zrow = const.tile([P, 2], F32)
        idx = const.tile([P, NCH, 2, 2], I32)

        nc.gpsimd.iota(pid[:], pattern=[[0, 1]], base=0, channel_multiplier=1)
        make_identity(nc, ident[:])
        make_block_diagonal(nc, ones4[:], 4)
        ctx.enter_context(tc.manual_schedule())

        def step_constants():
            for k in range(NS):
                nc.vector.memset(thr[:, k:k + 1], STEPS[k])
            for l in range(2):
                for e in range(2):
                    at = []
                    for k in range(LEV):
                        row = l * N_OK[k] + (TOP if k == 5 else 0) - e * (SIZES[k] - 1)
                        at.append(10.0 * row + 2.0 * min(k, TAB - 1))
                    for k in range(NS):
                        nc.vector.memset(gain[T * l:P, e, k:k + 1], at[k] - (at[k - 1] if k > 0 else 0.0))
            low = const.tile([P, 1], I32)
            nc.vector.tensor_single_scalar(out=low[:], in_=pid[:], scalar=15, op=ALU.bitwise_and)
            for i in range(2):
                s = 1.0 - 2.0 * i
                nc.vector.tensor_scalar(out=zrow[:, i:i + 1], in0=low[:], scalar1=10.0 * s, scalar2=(20.0 * N_OK[3] + 6.0) * s, op0=ALU.mult, op1=ALU.add)

        NQ = NCH * 2
        fl = const.tile([P, NQ, 2], F32)
        ln = const.tile([P, NQ], F32)
        wanted = const.tile([P, NQ, 2], F32)
        step = const.tile([P, NS, NQ], F32)
        part = const.tile([P, 2, NS, NQ], F32)

        def window_ends():
            whole = const.tile([P, NQ, 2], I32)
            nc.vector.tensor_scalar(out=whole[:].rearrange("p q e -> p (q e)"), in0=seg_bf[:].rearrange("p j h e -> p (j h e)"),
                                    scalar1=0.0, scalar2=-0.498, op0=ALU.max, op1=ALU.add)
            nc.vector.tensor_scalar(out=fl[:].rearrange("p q e -> p (q e)"), in0=whole[:].rearrange("p q e -> p (q e)"),
                                    scalar1=float(T - 1), scalar2=None, op0=ALU.min)
            nc.vector.tensor_tensor(out=ln[:], in0=fl[:, :, 1], in1=fl[:, :, 0], op=ALU.subtract)
            nc.vector.tensor_scalar(out=wanted[:, :, 0], in0=ln[:], scalar1=0.0, scalar2=None, op0=ALU.is_ge)

        def window_steps():
            nc.vector.tensor_tensor(out=step[:], in0=ln[:].unsqueeze(1).to_broadcast([P, NS, NQ]),
                                    in1=thr[:].unsqueeze(2).to_broadcast([P, NS, NQ]), op=ALU.is_ge)
            for e in range(2):
                nc.vector.tensor_tensor(out=part[:, e, :, :], in0=step[:],
                                        in1=gain[:, e, :].unsqueeze(2).to_broadcast([P, NS, NQ]), op=ALU.mult)

        def window_rows():
            total = const.tile([P, 2, NQ], F32)
            nc.vector.tensor_reduce(out=total[:].rearrange("p e q -> p (e q)"), in_=part[:].rearrange("p e k q -> p e q k"),
                                    axis=AX.X, op=ALU.add)
            size = const.tile([P, NQ], F32)
            nc.vector.tensor_tensor(out=size[:], in0=total[:, 0, :], in1=total[:, 1, :], op=ALU.subtract)
            nc.vector.scalar_tensor_tensor(out=fl[:], in0=fl[:], scalar=10.0, in1=total[:].rearrange("p e q -> p q e"), op0=ALU.mult, op1=ALU.add)
            nc.vector.scalar_tensor_tensor(out=wanted[:, :, 1], in0=ln[:], scalar=10.0, in1=size[:], op0=ALU.mult, op1=ALU.is_gt)
            nc.vector.scalar_tensor_tensor(out=fl[:], in0=fl[:], scalar=zrow[:, 1:2], in1=wanted[:], op0=ALU.add, op1=ALU.mult)
            second = fl[:].rearrange("p (j h) e -> p j h e", h=2)[:, SLOT_B + 1:SLOT_B + FOUR:2, :, :]
            nc.vector.tensor_scalar(out=second, in0=second, scalar1=float(2 * TAB * P), scalar2=None, op0=ALU.add)
            for h in range(2):
                nc.vector.tensor_scalar(out=idx[:, :, h, :], in0=fl[:].rearrange("p (j h) e -> p j h e", h=2)[:, :, h, :],
                                        scalar1=zrow[:, 0:1], scalar2=float(h), op0=ALU.add, op1=ALU.add)

        wstage = ctx.enter_context(tc.tile_pool(name="wstage", bufs=1))
        w_sb = wstage.tile([P, NM, C], BF16)
        nc.scalar.dma_start(out=seg_bf[:].rearrange("p j h e -> p j (h e)"), in_=segments.rearrange("(j l) n s -> (l n) j s", l=2))
        for mp in range(NM // 2):
            nc.sync.dma_start(out=w_sb[:, 2 * mp:2 * mp + 2, :],
                              in_=w_lr.rearrange("(p m) k -> p m k", m=NM)[:, 2 * mp:2 * mp + 2, :])
            if mp == 0:
                load_piece(0)
        load_piece(1)
        for i, v in enumerate((b_lr, g_lr, be_lr)):
            nc.gpsimd.dma_start(out=vec_bf[i][:], in_=v.rearrange("(p m) -> p m", m=NM))
        for k in range(1, TAB):
            used = ZERO if k == TAB - 1 else 2 * N_OK[k]
            nc.vector.memset(tab[:, k - 1, :, :, used:P], 0.0)

        w_words = w_sb[:].bitcast(F32).rearrange("p m (q u) -> p m q u", u=2)
        w_grp = wstage.tile([P, NM, P, 4], BF16, align_bytes=64)
        w_grp32 = w_grp[:].bitcast(F32)

        def quantise_w(hb):
            ms = slice(4 * hb, 4 * hb + 4)
            nc.vector.quantize_mx(out=w_codes[:, ms, :].rearrange("p m c -> p (m c)").bitcast(FP8X4),
                                  scales=w_scales[:, ms, :].rearrange("p m c -> p (m c)"),
                                  in_=w_grp[:, ms, :, :].rearrange("p m c j -> p (m c j)"))

        for mp in range(NM // 2):
            wt = tpsum.tile([P, 4, P], F32, name="wt", tag="tp")
            for i in range(2):
                for u in range(2):
                    nc.tensor.transpose(wt[:, 2 * i + u, :], w_words[:, 2 * mp + i, :, u], ident[:])
            nc.scalar.copy(out=w_grp32[:, 2 * mp, :, :], in_=wt[:, 0:2, :].rearrange("p u r -> p r u"))
            nc.scalar.copy(out=w_grp32[:, 2 * mp + 1, :, :], in_=wt[:, 2:4, :].rearrange("p u r -> p r u"))

        cc = const.tile([P, 2], F32)
        cg = const.tile([P, 2], F32)

        def norm_constants():
            bsq = const.tile([P, NM], F32)
            nc.vector.tensor_tensor(out=bsq[:], in0=beta, in1=beta, op=ALU.mult)
            nc.vector.tensor_reduce(out=cc[:, 0:1], in_=beta, axis=AX.X, op=ALU.add)
            nc.vector.tensor_reduce(out=cc[:, 1:2], in_=bsq[:], axis=AX.X, op=ALU.add)
            cg_ps = opsum.tile([P, 2], F32, name="cg_ps", tag="op")
            nc.tensor.matmul(out=cg_ps[:], lhsT=ones4[:], rhs=cc[:], start=True, stop=True)
            live["cg_ps"] = cg_ps

        fpool = ctx.enter_context(tc.tile_pool(name="fpool", bufs=2))
        late = ctx.enter_context(tc.tile_pool(name="late", bufs=LATE))
        rpool = ctx.enter_context(tc.tile_pool(name="rpool", bufs=2))
        gpool = ctx.enter_context(tc.tile_pool(name="gpool", bufs=2))
        opool = ctx.enter_context(tc.tile_pool(name="opool", bufs=2))

        def slot_of(pos):
            x, second = (pos // 2 % 2, pos % 2) if pos < FOUR else (pos % 2, 0)
            return (out_0, out_1)[x], second

        def slot_store(pos):
            o, second = slot_of(pos)
            return o[SLOT_B * second:SLOT_B * (second + 1)].rearrange("b (x c) t -> (b x) (c t)", c=16).rearrange("(r k) w -> r k w", k=TAB)

        def slot_rows(pos):
            o, second = slot_of(pos)
            return o[0:SLOT_B * (second + 1)].rearrange("b (x c) t -> (b x) (c t)", c=8)

        def mx_passes(y, pos, hb):
            cols = slice(P * order[pos], P * order[pos] + P)
            for i in range(4):
                m = 4 * hb + i
                nc.tensor.matmul_mx(out=y[:, i, :], lhsT=w_codes[:, m, :].bitcast(FP8X4), lhsT_scale=w_scales[:, m, :],
                                    rhs=x_codes[:, cols].bitcast(FP8X4), rhs_scale=x_scales[:, cols],
                                    start=True, stop=True)

        def group_of(pos):
            for q in range(len(pieces)):
                p0 = first_use(q)
                if p0 <= pos < p0 + pieces[q][1] // 2:
                    return q, 2 * (pos - p0)

        def squares(pos):
            if pos >= NCH:
                return
            q, bi = group_of(pos)
            if bi == 0:
                live[("terms", q)] = small.tile([P, NM + 2, 8], F32, name="terms", tag="terms")
                live[("s1", q)] = small.tile([P, NM, 8], F32, name="s1", tag="s1")
            terms = live[("terms", q)]
            ys = []
            for hb in range(2):
                y = ypsum.tile([P, 4, P], F32, name="y%d" % hb, tag="y%d" % hb)
                mx_passes(y, pos, hb)
                ys.append(y)
            for hb in range(2):
                nc.vector.tensor_reduce(out=live[("s1", q)][:, 4 * hb:4 * hb + 4, bi:bi + 2],
                                        in_=ys[hb][:].rearrange("p m (l t) -> p m l t", l=2), axis=AX.X, op=ALU.add)
            for hb in range(2):
                junk = small.tile([P, 4, T], F32, name="junk", tag="junk")
                for l in range(2):
                    nc.scalar.activation(out=junk[:], in_=ys[hb][:, :, T * l:T * l + T], func=ACT.Square,
                                         accum_out=terms[:, NM + hb, bi + l:bi + l + 1])

        def norm_steps(q):
            nb = pieces[q][1]
            full = [P, NM, nb]
            terms = live[("terms", q)]
            s1 = live[("s1", q)]
            rs = small.tile([P, 16], F32, name="rs", tag="rs")
            st = opsum.tile([P, 16], F32, name="st", tag="op")
            mv = small.tile([P, 2, 8], F32, name="mv", tag="mv")
            var = small.tile([P, 8], F32, name="var", tag="var")
            std = small.tile([P, 8], F32, name="std", tag="std")
            rstd = small.tile([P, 8], F32, name="rstd", tag="rstd")
            sc = small.tile([P, NM, 8], F32, name="sc", tag="sc")
            sh = small.tile([P, NM, 8], F32, name="sh", tag="sh")
            live[("sc", q)] = sc
            live[("sh", q)] = sh

            def bias_terms():
                nc.vector.scalar_tensor_tensor(out=terms[:, 0:NM, 0:nb], in0=s1[:, :, 0:nb], scalar=2.0,
                                               in1=beta.unsqueeze(2).to_broadcast(full), op0=ALU.mult, op1=ALU.mult)

            def over_tiles(part, src):
                nc.vector.tensor_reduce(out=rs[:, part * nb:part * nb + nb], in_=src.rearrange("p m b -> p b m"), axis=AX.X, op=ALU.add)

            def squares_over_tiles():
                over_tiles(1, terms[:, :, 0:nb])
                nc.tensor.matmul(out=st[:, 0:2 * nb], lhsT=ones4[:], rhs=rs[:, 0:2 * nb], start=True, stop=True)

            def moments():
                nc.vector.scalar_tensor_tensor(out=mv[:, :, 0:nb], in0=st[:, 0:2 * nb].rearrange("p (s b) -> p s b", s=2),
                                               scalar=1.0 / 2048.0, in1=cg[:].unsqueeze(2).to_broadcast([P, 2, nb]),
                                               op0=ALU.mult, op1=ALU.add)

            def mean_squared():
                nc.vector.tensor_tensor(out=var[:, 0:nb], in0=mv[:, 0, 0:nb], in1=mv[:, 0, 0:nb], op=ALU.mult)

            def deviation():
                nc.vector.scalar_tensor_tensor(out=var[:, 0:nb], in0=mv[:, 1, 0:nb], scalar=EPS, in1=var[:, 0:nb],
                                               op0=ALU.add, op1=ALU.subtract)
                nc.scalar.activation(out=std[:, 0:nb], in_=var[:, 0:nb], func=ACT.Sqrt)

            def shift_a():
                nc.vector.tensor_tensor(out=sh[:, :, 0:nb], in0=beta.unsqueeze(2).to_broadcast(full),
                                        in1=mv[:, 0, 0:nb].unsqueeze(1).to_broadcast(full), op=ALU.subtract)

            def inverse():
                nc.vector.reciprocal(out=rstd[:, 0:nb], in_=std[:, 0:nb])

            def scale():
                nc.vector.tensor_tensor(out=sc[:, :, 0:nb], in0=gamma.unsqueeze(2).to_broadcast(full),
                                        in1=rstd[:, 0:nb].unsqueeze(1).to_broadcast(full), op=ALU.mult)

            def shift_b():
                nc.vector.tensor_tensor(out=sh[:, :, 0:nb], in0=sh[:, :, 0:nb], in1=sc[:, :, 0:nb], op=ALU.mult)

            def shift_c():
                nc.vector.tensor_tensor(out=sh[:, :, 0:nb], in0=sh[:, :, 0:nb], in1=shift0.unsqueeze(2).to_broadcast(full), op=ALU.add)

            return [bias_terms, lambda: over_tiles(0, s1[:, :, 0:nb]), squares_over_tiles,
                    moments, mean_squared, deviation, shift_a, inverse, scale, shift_b, shift_c]

        def next_step():
            if live["steps"]:
                live["steps"].pop(0)()

        def all_steps():
            while live["steps"]:
                next_step()

        def main_mx(pos):
            ys = []
            for hb in range(2):
                y = ypsum.tile([P, 4, P], F32, name="y%d" % hb, tag="y%d" % hb)
                mx_passes(y, pos, hb)
                ys.append(y)
            live[("y", pos)] = ys

        def apply_norm(pos, hb):
            if hb == 0:
                live[("f", pos)] = fpool.tile([P, 2, 4, P], F32, name="f", tag="f")
            f = live[("f", pos)]
            ys = live[("y", pos)]
            q, bi = group_of(pos)
            sc = live[("sc", q)]
            sh = live[("sh", q)]
            for i in range(4):
                m = 4 * hb + i
                for l in range(2):
                    b = bi + l
                    nc.scalar.activation(out=f[:, m % 2, m // 2, T * l:T * l + T], in_=ys[hb][:, i, T * l:T * l + T],
                                         func=ACT.Relu, bias=sh[:, m, b:b + 1], scale=sc[:, m, b:b + 1])

        def send(x, dst, src):
            if held[x] is None:
                nc.sync.dma_start(out=dst, in_=src)
            else:
                held[x].append((dst, src))

        def give_up_slot(x):
            for dst, src in held[x]:
                nc.sync.dma_start(out=dst, in_=src)
            held[x] = None

        def copy_feat(pos, l):
            if l == 0:
                if order[pos] < LATE:
                    live[("f2", pos)] = late.tile([P, 2, NM, T], F32, name="f2_late", tag="f2_late")
                else:
                    live[("f2", pos)] = opool.tile([P, 2, NM, T], F32, name="f2", tag="f2")
            out = live[("f2", pos)][:, l, :, :].rearrange("p (j mm) t -> p j mm t", mm=2)
            src = live[("f", pos)][:, :, :, T * l:T * l + T].rearrange("p mm j t -> p j mm t")
            nc.scalar.copy(out=out, in_=src)

        def store_feat(pos):
            j = order[pos]
            dst = out_0[2 * j:2 * j + 2].rearrange("l (p m) t -> p l (m t)", m=NM)
            src = live[("f2", pos)][:].rearrange("p l m t -> p l (m t)")
            if j < LATE:
                send(0, dst, src)
            else:
                nc.sync.dma_start(out=dst, in_=src)

        def view(k, mm):
            if k == 5:
                cols = tab[:, 3, mm, :, TOP:TOP + 2 * N_OK[5]]
            else:
                cols = tab[:, k - 1, mm, :, 0:2 * N_OK[k]]
            return cols.rearrange("p j (l t) -> p j l t", l=2)

        def window(out, in_, shift, n):
            nc.vector.tensor_tensor(out=out, in0=in_[:, :, :, 0:n], in1=in_[:, :, :, shift:shift + n], op=ALU.max)
            next_step()

        def pairs_up(pos):
            for mm in range(2):
                window(pairs[:, mm, :, :].rearrange("p j (l t) -> p j l t", l=2),
                       live[("f", pos)][:, mm, :, :].rearrange("p j (l t) -> p j l t", l=2), 1, T - 1)

        def level_up(pos, k):
            for mm in range(2):
                if k == 0:
                    window(view(1, mm), pairs[:, mm, :, :].rearrange("p j (l t) -> p j l t", l=2), 1, N_OK[1])
                else:
                    window(view(k + 1, mm), view(k, mm), SIZES[k], N_OK[k + 1])

        def rows_out(pos, k):
            u, first = k // 2, k % 2 == 0
            if first:
                n = 2 if k < TAB - 1 else 1
                live[("r", pos, u)] = rpool.tile([P, n, 2, 2, 4, 64], F32, name="r%d" % u, tag="r%d" % u)
            r = live[("r", pos, u)]
            for mm in range(2):
                tp = tpsum.tile([P, 4, P], F32, name="tp", tag="tp")
                for j in range(4):
                    src = live[("f", pos)][:, mm, j, :] if k == 0 else tab[:, k - 1, mm, j, :]
                    nc.tensor.transpose(tp[:, j, :], src, ident[:])
                dst = r[:, k % 2, :, mm, :, :]
                rows = tp[:].rearrange("p j (h q) -> p h j q", h=2)
                if k == TAB - 2 and mm == 1:
                    live["late_copy"] = (dst, rows)
                elif k == TAB - 1:
                    nc.vector.tensor_copy(out=dst, in_=rows)
                else:
                    nc.scalar.copy(out=dst, in_=rows)

        def late_copy():
            dst, rows = live["late_copy"]
            nc.vector.tensor_copy(out=dst, in_=rows)

        def store_rows(pos, u):
            r = live[("r", pos, u)]
            nc.sync.dma_start(out=slot_store(pos)[:, 2 * u:min(2 * u + 2, TAB), :],
                              in_=r[:].rearrange("p k h mm j q -> p k (h mm j q)"))

        def gathers(pos):
            j = order[pos]
            got = [gpool.tile([P, 2, C], F32, name="g%d" % e, tag="g%d" % e, bufs=3) for e in range(2)]
            for h in range(2):
                for e in range(2):
                    nc.gpsimd.indirect_dma_start(out=got[e][:, h, :], out_offset=None, in_=slot_rows(pos),
                                                 in_offset=bass.IndirectOffsetOnAxis(ap=idx[:, j, h, e:e + 1], axis=0))
            live[("g", pos)] = got

        def window_max(pos):
            gc = gpool.tile([P, NM, 2, 64], F32, name="gc", tag="gc")
            got = [x[:].rearrange("p h (m q) -> p h m q", m=NM) for x in live[("g", pos)]]
            nc.vector.tensor_tensor(out=gc[:].rearrange("p m h q -> p h m q"), in0=got[0], in1=got[1], op=ALU.max)
            live[("gc", pos)] = gc

        def pooled_out(pos, hb):
            j = order[pos]
            is_late = j < LATE
            gc = live[("gc", pos)]
            if hb == 0:
                if is_late:
                    live[("o", pos)] = late.tile([P, 2, NM, T], F32, name="o_late", tag="o_late")
                else:
                    live[("o", pos)] = opool.tile([P, 2, NM, T], F32, name="o", tag="o")
            o = live[("o", pos)]
            op = opsum.tile([P, 4, P], F32, name="op", tag="op")
            for i in range(4):
                nc.tensor.transpose(op[:, i, :], gc[:, 4 * (i % 2) + 2 * hb + i // 2, :, :].rearrange("p h q -> p (h q)"), ident[:])
            nc.scalar.copy(out=o[:, :, 4 * hb:4 * hb + 4, :], in_=op[:].rearrange("p m (l n) -> p l m n", l=2))

        def store_pooled(pos):
            j = order[pos]
            dst = out_1[2 * j:2 * j + 2].rearrange("l (p m) n -> p l (m n)", m=NM)
            src = live[("o", pos)][:].rearrange("p l m n -> p l (m n)")
            if j < LATE:
                send(1, dst, src)
            else:
                nc.sync.dma_start(out=dst, in_=src)

        def group_all(q):
            for b in range(0, pieces[q][1], 2):
                group_piece(q, b)

        def one_round(a):
            c = a - 1
            w = c - 3
            first = a < NCH
            second = 0 <= c < NCH
            third = 0 <= w < NCH
            early = {1: (1, 2), 2: (2, 3), 3: (3, 5)}

            def at(q, stage):
                return early[q][stage] if q in early else first_use(q) - (5, 1)[stage]

            def due(stage):
                return [q for q in range(1, len(pieces)) if at(q, stage) == a]

            if second:
                rows_out(c, 0)
                pairs_up(c)
            if a > 1:
                squares(min(2 * a - 1, a + 4))
            for q in range(1, len(pieces)):
                if q in early and a == at(q, 0):
                    group_all(q)
                if q not in early:
                    b = 2 * (a - at(q, 0)) + pieces[q][1] - 2
                    if 0 <= b < pieces[q][1]:
                        group_piece(q, b)
            for q in due(1):
                live["steps"] += norm_steps(q)
            if second:
                level_up(c, 0)
                rows_out(c, 1)
                store_rows(c, 0)
            if second:
                level_up(c, 1)
                rows_out(c, 2)
            for q in due(0):
                quantise_piece(q)
            if third:
                window_max(w)
                if w >= NCH - 2:
                    give_up_slot(w % 2)
            if first:
                main_mx(a)
            if second:
                level_up(c, 2)
                rows_out(c, 3)
            if any(first_use(q) == a for q in range(1, len(pieces))):
                all_steps()
            if first:
                apply_norm(a, 0)
                apply_norm(a, 1)
            if third:
                pooled_out(w, 0)
                pooled_out(w, 1)
            if second:
                level_up(c, 3)
                level_up(c, 4)
                late_copy()
                store_rows(c, 1)
                copy_feat(c, 0)
                copy_feat(c, 1)
                rows_out(c, 4)
                store_rows(c, 2)
                gathers(c)
            if 1 <= a <= 4:
                squares(2 * a)
            if third:
                store_pooled(w)
            if second:
                store_feat(c)
            for q in range(2, len(pieces)):
                if a == (max(first_use(q) - 10, 1) if q not in early else q - 2):
                    load_piece(q)

        step_constants()
        warm = const.tile([P, 1], F32)
        nc.scalar.activation(out=warm[:], in_=thr[:, 1:2], func=ACT.Sqrt)
        window_ends()
        group_all(0)
        quantise_piece(0)
        norm_constants()
        quantise_w(0)
        quantise_w(1)
        squares(0)
        squares(1)
        live["steps"] = norm_steps(0)
        next_step()
        next_step()
        nc.vector.tensor_scalar(out=cg[:], in0=live["cg_ps"][:], scalar1=64.0 / 2048.0, scalar2=None, op0=ALU.mult)
        window_steps()
        all_steps()
        window_rows()
        for a in range(NCH + 4):
            one_round(a)
